import numpy as np
import ml_dtypes


def mxq(x, axis, fmt="e4m3"):
    dtype, down = {"e4m3": (ml_dtypes.float8_e4m3fn, 7), "e5m2": (ml_dtypes.float8_e5m2, 14)}[fmt]
    v = np.moveaxis(np.asarray(x, np.float32).astype(ml_dtypes.bfloat16).astype(np.float64), axis, -1)
    blocks = v.reshape(v.shape[:-1] + (-1, 32))
    amax = np.abs(blocks).max(-1, keepdims=True)
    byte = np.maximum(np.where(amax > 0, np.frexp(amax)[1] - 1 + 127, 0) - down, 1)
    scale = np.exp2(byte - 127.0)
    codes = (blocks / scale).astype(np.float32).astype(dtype).astype(np.float64)
    return np.moveaxis((codes * scale).reshape(v.shape), -1, axis)


WIDE = False


def mx_kscale(k):
    if not WIDE:
        return np.ones(k)
    levels = np.array([10, -10, 5, -5, 0])
    if k % 512:
        return np.exp2(np.random.permutation(np.resize(levels, k // 32))).repeat(32)
    a = np.empty((k // 512, 16))
    for p in range(k // 512):
        a[p, :8] = np.random.permutation(np.resize(levels, 8))
        for g in range(8):
            far = levels[np.abs(levels - a[p, g]) >= 10]
            a[p, g + 8] = far[np.random.randint(len(far))]
    return np.exp2(a.ravel()).repeat(32)


BF16 = ml_dtypes.bfloat16


def bf(x):
    return np.asarray(x, np.float32).astype(BF16)


def f64(x):
    return np.asarray(x).astype(np.float64)


B, C, M, O, H, W = 4, 512, 512, 512, 32, 32
H2, W2 = H // 2, W // 2
KS = 3
PAD = KS // 2
BN_EPS = 1e-5


def haar_ll(x):
    a = x[:, :, 0::2, 0::2]
    b = x[:, :, 0::2, 1::2]
    c = x[:, :, 1::2, 0::2]
    d = x[:, :, 1::2, 1::2]
    return (a + b + c + d) * 0.5


def windows(u):
    up = np.pad(u, ((0, 0), (0, 0), (PAD, PAD), (PAD, PAD)))
    return np.stack([up[:, :, i:i + H2, j:j + W2] for i in range(KS) for j in range(KS)], axis=-1)


def setup_inputs():
    s, t = mx_kscale(C), mx_kscale(M)
    return {
        "x": bf(np.random.standard_normal((B, C, H, W)) * s[None, :, None, None]),
        "w_c1": bf(np.random.standard_normal((M, C)) / np.sqrt(C) * t[:, None] / s[None, :]),
        "b_c1": bf(np.random.standard_normal(M) * 0.3 * t),
        "w_q": bf(np.random.standard_normal((O, M)) / np.sqrt(M) / t[None, :]),
        "w_k": bf(np.random.standard_normal((O, M)) / np.sqrt(M) / t[None, :]),
        "w_v": bf(np.random.standard_normal((O, M)) / np.sqrt(M) / t[None, :]),
        "bn_gamma": bf(1.0 + 0.1 * np.random.standard_normal(O)),
        "bn_beta": bf(0.3 * np.random.standard_normal(O)),
        "prelu_a": bf(np.random.uniform(0.15, 0.35, (1,))),
    }


def reference(x, w_c1, b_c1, w_q, w_k, w_v, bn_gamma, bn_beta, prelu_a):
    ll = haar_ll(f64(x)).reshape(B, C, H2 * W2)
    y = f64(bf(mxq(f64(w_c1), 1, "e4m3") @ mxq(ll, 1, "e4m3"))) + f64(b_c1)[None, :, None]
    yq = mxq(y, 1, "e4m3")
    q = (mxq(f64(w_q), 1, "e4m3") @ yq).reshape(B, O, H2, W2)
    k = (mxq(f64(w_k), 1, "e4m3") @ yq).reshape(B, O, H2, W2)
    v = (mxq(f64(w_v), 1, "e4m3") @ yq).reshape(B, O, H2, W2)
    kw = windows(k)
    vw = windows(v)
    z = q[..., None] * kw
    e = np.exp(z - z.max(-1, keepdims=True))
    attn = e / e.sum(-1, keepdims=True)
    att = (attn * vw).sum(-1)
    m = att.mean(axis=(0, 2, 3), keepdims=True)
    var = att.var(axis=(0, 2, 3), keepdims=True)
    n = f64(bn_gamma)[None, :, None, None] * (att - m) / np.sqrt(var + BN_EPS) + f64(bn_beta)[None, :, None, None]
    return np.where(n >= 0, n, f64(prelu_a) * n)

@@ -1,0 +1,396 @@
+from contextlib import ExitStack
+
+import concourse.mybir as mybir
+from concourse.masks import make_identity
+
+F32 = mybir.dt.float32
+BF16 = mybir.dt.bfloat16
+I32 = mybir.dt.int32
+U8 = mybir.dt.uint8
+FP8X4 = mybir.dt.float8_e4m3fn_x4
+ALU = mybir.AluOpType
+ACT = mybir.ActivationFunctionType
+
+P = 128
+NB = 4
+NPIX = 1024
+ROW = 64
+STEPS = 8
+BN_EPS = 1e-5
+BANK_DT = BF16
+AHEAD = 3
+T_BURST = 6
+
+FLOPS = 4 * 2 * 512 * 512 * 1024
+
+
+def tile_merge_pa_kernel(tc, x, w_c1, b_c1, w_q, w_k, w_v, bn_gamma, bn_beta, prelu_a, out):
+    nc = tc.nc
+    with ExitStack() as ctx:
+        keep = ctx.enter_context(tc.tile_pool(name="keep", bufs=1))
+        mid = ctx.enter_context(tc.tile_pool(name="mid", bufs=1))
+
+        ident = keep.tile([P, P], F32, name="ident")
+        make_identity(nc, ident[:])
+
+        w_codes = []
+        w_scales = []
+        for i in range(4):
+            wct = keep.tile([P, 512], I32, name="w_codes%d" % i, align_bytes=64)
+            wst = keep.tile([P, 512], U8, name="w_scales%d" % i, align_bytes=64)
+            w_codes.append(wct)
+            w_scales.append(wst)
+        ll_codes = keep.tile([P, NPIX], I32, name="ll_codes", align_bytes=64)
+        ll_scales = keep.tile([P, NPIX], U8, name="ll_scales", align_bytes=64)
+        y_codes = []
+        y_scales = []
+        for d in range(3):
+            yct = keep.tile([P, NPIX + 2 * ROW], I32, name="y_codes%d" % d, align_bytes=64)
+            yst = keep.tile([P, NPIX + 2 * ROW], U8, name="y_scales%d" % d, align_bytes=64)
+            for c0 in (0, ROW + NPIX):
+                nc.vector.memset(yct[:, c0:c0 + ROW], 0)
+                nc.vector.memset(yst[:, c0:c0 + ROW].bitcast(I32), 0)
+            y_codes.append(yct)
+            y_scales.append(yst)
+
+        att = keep.tile([P, 4, NPIX], F32, name="att")
+        stats = keep.tile([P, 4, STEPS, 6], F32, name="stats")
+
+        bias_bf = keep.tile([P, 4], BF16, name="bias_bf")
+        gam_bf = keep.tile([P, 4], BF16, name="gam_bf")
+        bet_bf = keep.tile([P, 4], BF16, name="bet_bf")
+        a_bf = keep.tile([P, 1], BF16, name="a_bf")
+        nc.gpsimd.dma_start(out=bias_bf[:], in_=b_c1.rearrange("(p t) -> p t", t=4))
+        nc.gpsimd.dma_start(out=gam_bf[:], in_=bn_gamma.rearrange("(p t) -> p t", t=4))
+        nc.gpsimd.dma_start(out=bet_bf[:], in_=bn_beta.rearrange("(p t) -> p t", t=4))
+        nc.gpsimd.dma_start(out=a_bf[:], in_=prelu_a.partition_broadcast(P))
+        a_col = keep.tile([P, 1], F32, name="a_col")
+        nc.vector.tensor_copy(out=a_col[:], in_=a_bf[:])
+        zeros_bf = keep.tile([P, P], BF16, name="zeros_bf")
+        nc.vector.memset(zeros_bf[:], 0.0)
+        bias_full = keep.tile([P, P, 4], BF16, name="bias_full")
+        for t in range(4):
+            nc.vector.tensor_scalar(out=bias_full[:, :, t], in0=zeros_bf[:], scalar1=bias_bf[:, t:t + 1],
+                                    scalar2=None, op0=ALU.add)
+
+        ll = mid.tile([P, NPIX, 4], BF16, name="ll", align_bytes=64)
+        y_mid = mid.tile([P, NPIX, 4], BF16, name="y_mid", align_bytes=64)
+        y_left = mid.tile([P, NPIX, 4], BF16, name="y_left", align_bytes=64)
+        y_right = mid.tile([P, NPIX, 4], BF16, name="y_right", align_bytes=64)
+        nc.gpsimd.memset(y_left[:], 0.0)
+        nc.gpsimd.memset(y_right[:], 0.0)
+        ll_by_image = ll[:].rearrange("p (y b x) j -> p b y x j", b=NB, x=16)
+        ll_flat = ll[:].rearrange("p c j -> p (c j)")
+        lefts = y_left[:].rearrange("p (g x) t -> p g (x t)", x=16)
+        mids = y_mid[:].rearrange("p (g x) t -> p g (x t)", x=16)
+        rights = y_right[:].rearrange("p (g x) t -> p g (x t)", x=16)
+
+        def quant_ll(h):
+            nc.vector.quantize_mx(out=ll_codes[:, 512 * h:512 * (h + 1)].bitcast(FP8X4),
+                                  scales=ll_scales[:, 512 * h:512 * (h + 1)],
+                                  in_=ll_flat[:, 2048 * h:2048 * (h + 1)])
+
+        def first_conv(bank, r):
+            cols = slice(P * r, P * (r + 1))
+            for t in range(4):
+                nc.tensor.matmul_mx(out=bank[:, t, :],
+                                    lhsT=w_codes[0][:, P * t:P * (t + 1)].bitcast(FP8X4),
+                                    lhsT_scale=w_scales[0][:, P * t:P * (t + 1)],
+                                    rhs=ll_codes[:, cols].bitcast(FP8X4), rhs_scale=ll_scales[:, cols],
+                                    start=True, stop=True)
+
+        def add_bias(bank, r):
+            nc.vector.tensor_tensor(out=y_mid[:, P * r:P * (r + 1), :], in0=bank[:].rearrange("p t n -> p n t"),
+                                    in1=bias_full[:], op=ALU.add)
+
+        def shift_copies(h):
+            g0 = 32 * h
+            nc.scalar.copy(out=lefts[:, g0:g0 + 32, 4:64], in_=mids[:, g0:g0 + 32, 0:60])
+            nc.scalar.copy(out=rights[:, g0:g0 + 32, 0:60], in_=mids[:, g0:g0 + 32, 4:64])
+
+        def quant_y(h):
+            c0 = ROW + 512 * h
+            for d, ysrc in enumerate((y_left, y_mid, y_right)):
+                nc.vector.quantize_mx(out=y_codes[d][:, c0:c0 + 512].bitcast(FP8X4),
+                                      scales=y_scales[d][:, c0:c0 + 512],
+                                      in_=ysrc[:].rearrange("p c j -> p (c j)")[:, 2048 * h:2048 * (h + 1)])
+
+        with tc.tile_pool(name="early", bufs=1) as early, tc.psum_pool(name="psh", bufs=2) as psh:
+            weights = (w_c1, w_k, w_q, w_v)
+            x_sb = []
+            w_sb = []
+            for i in range(4):
+                xt = early.tile([P, 4, 1024], BF16, name="x_sb%d" % i)
+                x_sb.append(xt)
+                wt = early.tile([P, 4, 512], BF16, name="w_sb%d" % i)
+                w_sb.append(wt)
+
+            def load_w(i):
+                nc.sync.dma_start(out=w_sb[i][:], in_=weights[i].rearrange("(c r) k -> c r k", r=4))
+
+            def load_x(b, h):
+                nc.sync.dma_start(out=x_sb[b][:, :, 512 * h:512 * (h + 1)],
+                                  in_=x[b].rearrange("(p j) h w -> p j (h w)", j=4)[:, :, 512 * h:512 * (h + 1)])
+
+            load_w(0)
+            for b in range(NB):
+                load_x(b, 0)
+            for i in range(1, 4):
+                load_w(i)
+            for b in range(NB):
+                load_x(b, 1)
+
+            def haar(b, h):
+                rows = x_sb[b][:, :, 512 * h:512 * (h + 1)].rearrange("p j (i a w) -> p j i a w", a=2, w=32)
+                s1 = early.tile([P, 4, 8, 32], F32, name="s1", tag="s1", bufs=2)
+                nc.vector.tensor_tensor(out=s1[:], in0=rows[:, :, :, 0, :], in1=rows[:, :, :, 1, :], op=ALU.add)
+                pairs = s1[:].rearrange("p j i (x e) -> p (j i x) e", e=2)
+                s2 = early.tile([P, 512], F32, name="s2", tag="s2", bufs=2)
+                nc.vector.tensor_tensor(out=s2[:], in0=pairs[:, :, 0], in1=pairs[:, :, 1], op=ALU.add)
+                nc.scalar.activation(out=ll_by_image[:, b, 8 * h:8 * (h + 1)],
+                                     in_=s2[:].rearrange("p (j y x) -> p y x j", j=4, x=16),
+                                     func=ACT.Copy, scale=0.5)
+
+            def prep_weight(i):
+                words = w_sb[i][:].bitcast(F32)
+                grouped = early.tile([P, 2048], BF16, name="grouped", tag="grouped", bufs=2, align_bytes=64)
+                gwords = grouped[:].bitcast(F32).rearrange("p (r c u) -> p r c u", r=4, u=2)
+                for h in range(2):
+                    wT = psh.tile([P, 2, 2, P], F32, name="wT", tag="wT")
+                    for rr in range(2):
+                        for u in range(2):
+                            nc.tensor.transpose(wT[:, rr, u, :], words[:, 2 * h + rr, u:256:2], ident[:])
+                    nc.scalar.copy(out=gwords[:, 2 * h:2 * h + 2], in_=wT[:].rearrange("p r u c -> p r c u"))
+                nc.vector.quantize_mx(out=w_codes[i][:].bitcast(FP8X4), scales=w_scales[i][:], in_=grouped[:])
+
+            prep_weight(0)
+            for b in range(NB):
+                haar(b, 0)
+            quant_ll(0)
+            for r in range(4):
+                bank = psh.tile([P, 4, P], BANK_DT, name="bank", tag="bank")
+                first_conv(bank, r)
+                add_bias(bank, r)
+            for i in range(1, 4):
+                prep_weight(i)
+            shift_copies(0)
+            quant_y(0)
+            for b in range(NB):
+                haar(b, 1)
+
+        with tc.tile_pool(name="main", bufs=2) as main, tc.psum_pool(name="psm", bufs=1) as psm:
+            zs = {}
+            evs = {}
+            nums = {}
+            dens = {}
+            q_sbs = {}
+            rds = {}
+            banks = {}
+
+            def ok(s):
+                return 0 <= s < STEPS
+
+            def conv(dst, s, j, wi):
+                c0 = ROW + P * s + ROW * (j // 3 - 1)
+                d = j % 3
+                nc.tensor.matmul_mx(out=dst, lhsT=y_codes[d][:, c0:c0 + P].bitcast(FP8X4),
+                                    lhsT_scale=y_scales[d][:, c0:c0 + P],
+                                    rhs=w_codes[wi][:].bitcast(FP8X4), rhs_scale=w_scales[wi][:],
+                                    start=True, stop=True)
+
+            pe_list = [("q", 0, 0)] + [("k", 0, j) for j in range(AHEAD)]
+            for s in range(STEPS + 2):
+                mms = []
+                if ok(s):
+                    mms.extend([("k", s, j) for j in range(AHEAD, 9)])
+                if ok(s + 1):
+                    mms.append(("q", s + 1, 0))
+                if s == 1:
+                    mms.extend([("c", r, 0) for r in range(4, 8)])
+                sums = []
+                if ok(s - 2):
+                    mms.extend([("v", s - 2, j) for j in range(AHEAD, 9)])
+                    sums = [("F", s - 2, i) for i in range(36)]
+                for n, tok in enumerate(mms):
+                    pe_list.append(tok)
+                    if n % 2 == 1:
+                        pe_list.extend(sums[:T_BURST])
+                        sums = sums[T_BURST:]
+                pe_list.extend(sums)
+                if ok(s + 1):
+                    pe_list.extend([("k", s + 1, j) for j in range(AHEAD)])
+                if ok(s - 1):
+                    pe_list.extend([("v", s - 1, j) for j in range(AHEAD)])
+                if ok(s - 2):
+                    pe_list.extend([("G", s - 2, i) for i in range(36)])
+
+            def add_up(dst, src, i):
+                ob = i // 9
+                j = i % 9
+                nc.tensor.matmul(out=dst[:, ob, :], lhsT=src[:, j, P * ob:P * (ob + 1)], rhs=ident[:],
+                                 is_transpose=True, start=(j == 0), stop=(j == 8))
+
+            def emit_pe(tok):
+                kind, s, j = tok
+                if kind == "q":
+                    q_ps = psm.tile([P, 512], F32, name="q_ps", tag="k_ps", bufs=3)
+                    conv(q_ps[:], s, 4, 2)
+                    banks[tok] = q_ps
+                elif kind == "k":
+                    k_ps = psm.tile([P, 512], F32, name="k_ps", tag="k_ps", bufs=3)
+                    conv(k_ps[:], s, j, 1)
+                    banks[tok] = k_ps
+                elif kind == "v":
+                    v_ps = psm.tile([P, 512], F32, name="v_ps", tag="v_ps", bufs=3)
+                    conv(v_ps[:], s, j, 3)
+                    banks[tok] = v_ps
+                elif kind == "c":
+                    bank2 = psm.tile([P, 4, P], BANK_DT, name="bank2", tag="v_ps", bufs=3)
+                    first_conv(bank2, s)
+                    banks[tok] = bank2
+                elif kind == "F":
+                    if j == 0:
+                        den = psm.tile([P, 4, P], F32, name="den", tag="den", bufs=1)
+                        dens[s] = den
+                    add_up(dens[s], zs[s], j)
+                else:
+                    if j == 0:
+                        num = psm.tile([P, 4, P], F32, name="num", tag="num", bufs=1)
+                        nums[s] = num
+                    add_up(nums[s], evs[s], j)
+
+            done = set()
+            pos = [0]
+
+            def pump_to(tok):
+                while tok not in done:
+                    nxt = pe_list[pos[0]]
+                    pos[0] += 1
+                    emit_pe(nxt)
+                    done.add(nxt)
+
+            def q_copy(s):
+                pump_to(("q", s, 0))
+                q_sb = main.tile([P, 512], F32, name="q_sb", tag="q_sb")
+                nc.scalar.copy(out=q_sb[:], in_=banks[("q", s, 0)][:])
+                q_sbs[s] = q_sb
+
+            def scores(s):
+                z = main.tile([P, 9, 512], F32, name="z", tag="z", bufs=3)
+                zs[s] = z
+                for j in range(9):
+                    pump_to(("k", s, j))
+                    nc.vector.tensor_tensor(out=z[:, j, :], in0=q_sbs[s][:], in1=banks[("k", s, j)][:], op=ALU.mult)
+
+            def shift_by_max(s):
+                z = zs[s]
+                t1 = main.tile([P, 4, 512], F32, name="t1", tag="t1", bufs=1)
+                nc.vector.tensor_tensor(out=t1[:], in0=z[:, 0:4, :], in1=z[:, 4:8, :], op=ALU.max)
+                t2 = main.tile([P, 2, 512], F32, name="t2", tag="t2", bufs=1)
+                nc.vector.tensor_tensor(out=t2[:], in0=t1[:, 0:2, :], in1=t1[:, 2:4, :], op=ALU.max)
+                t3 = main.tile([P, 512], F32, name="t3", tag="t3", bufs=1)
+                nc.vector.tensor_tensor(out=t3[:], in0=t2[:, 0, :], in1=t2[:, 1, :], op=ALU.max)
+                m = main.tile([P, 512], F32, name="m", tag="m")
+                nc.vector.tensor_tensor(out=m[:], in0=t3[:], in1=z[:, 8, :], op=ALU.max)
+                for j in range(9):
+                    nc.gpsimd.tensor_tensor(out=z[:, j, :], in0=z[:, j, :], in1=m[:], op=ALU.subtract)
+
+            def exps(s, g):
+                z = zs[s]
+                nc.scalar.activation(out=z[:, 3 * g:3 * g + 3, :], in_=z[:, 3 * g:3 * g + 3, :], func=ACT.Exp)
+
+            def weigh(s, j0, j1):
+                if j0 == 0:
+                    ev = main.tile([P, 9, 512], F32, name="ev", tag="ev", bufs=2)
+                    evs[s] = ev
+                for j in range(j0, j1):
+                    pump_to(("v", s, j))
+                    nc.vector.tensor_tensor(out=evs[s][:, j, :], in0=zs[s][:, j, :], in1=banks[("v", s, j)][:],
+                                            op=ALU.mult)
+
+            def one_over_den(s):
+                pump_to(("F", s, 35))
+                lg = main.tile([P, 4, P], F32, name="lg", tag="lg")
+                nc.scalar.activation(out=lg[:], in_=dens[s][:], func=ACT.Ln)
+                rd = main.tile([P, 4, P], F32, name="rd", tag="rd")
+                nc.scalar.activation(out=rd[:], in_=lg[:], func=ACT.Exp, scale=-1.0)
+                rds[s] = rd
+
+            def divide(s):
+                pump_to(("G", s, 35))
+                cols = slice(P * s, P * (s + 1))
+                nc.vector.tensor_tensor(out=att[:, :, cols], in0=nums[s][:], in1=rds[s][:], op=ALU.mult)
+                for ob in range(4):
+                    nc.vector.bn_stats(out=stats[:, ob, s, :], in_=att[:, ob, cols])
+
+            warm = main.tile([P, 1], F32, name="warm", tag="warm", bufs=1)
+            with tc.manual_schedule():
+                q_copy(0)
+                for s in range(STEPS):
+                    scores(s)
+                    if s == 1:
+                        for r in range(4, 8):
+                            pump_to(("c", r, 0))
+                            add_bias(banks[("c", r, 0)], r)
+                    if s == 2:
+                        quant_y(1)
+                    if ok(s - 3):
+                        divide(s - 3)
+                    if ok(s - 2):
+                        weigh(s - 2, 0, 9)
+                    shift_by_max(s)
+                    if s == 0:
+                        quant_ll(1)
+                    if ok(s - 1):
+                        exps(s - 1, 0)
+                    if ok(s + 1):
+                        q_copy(s + 1)
+                    if ok(s - 1):
+                        exps(s - 1, 1)
+                    if s == 1:
+                        shift_copies(1)
+                    if ok(s - 1):
+                        exps(s - 1, 2)
+                    if ok(s - 2):
+                        one_over_den(s - 2)
+                divide(STEPS - 3)
+                exps(STEPS - 1, 0)
+                weigh(STEPS - 2, 0, 9)
+                one_over_den(STEPS - 2)
+                exps(STEPS - 1, 1)
+                exps(STEPS - 1, 2)
+                weigh(STEPS - 1, 0, 6)
+                divide(STEPS - 2)
+                weigh(STEPS - 1, 6, 9)
+                one_over_den(STEPS - 1)
+                nc.scalar.activation(out=warm[:], in_=rds[STEPS - 1][:, 0, 0:1], func=ACT.Sqrt)
+                divide(STEPS - 1)
+
+            mv = main.tile([P, 4, 2], F32, name="mv", tag="mv", bufs=1)
+            for ob in range(4):
+                nc.vector.bn_aggr(out=mv[:, ob, :], in_=stats[:, ob, :, :].rearrange("p s k -> p (s k)"))
+            ve = main.tile([P, 4], F32, name="ve", tag="ve", bufs=1)
+            nc.vector.tensor_scalar(out=ve[:], in0=mv[:, :, 1], scalar1=BN_EPS, scalar2=None, op0=ALU.add)
+            sd = main.tile([P, 4], F32, name="sd", tag="sd", bufs=1)
+            nc.scalar.activation(out=sd[:], in_=ve[:], func=ACT.Sqrt)
+            rstd = main.tile([P, 4], F32, name="rstd", tag="rstd", bufs=1)
+            nc.vector.reciprocal(out=rstd[:], in_=sd[:])
+            gain = main.tile([P, 4], F32, name="gain", tag="gain", bufs=1)
+            nc.vector.tensor_tensor(out=gain[:], in0=gam_bf[:], in1=rstd[:], op=ALU.mult)
+            mg = main.tile([P, 4], F32, name="mg", tag="mg", bufs=1)
+            nc.vector.tensor_tensor(out=mg[:], in0=mv[:, :, 0], in1=gain[:], op=ALU.mult)
+            shift = main.tile([P, 4], F32, name="shift", tag="shift", bufs=1)
+            nc.vector.tensor_tensor(out=shift[:], in0=bet_bf[:], in1=mg[:], op=ALU.subtract)
+            out_v = out.rearrange("b (c r) h w -> c r b (h w)", r=4)
+            for ob in range(4):
+                n = main.tile([P, NPIX], F32, name="n", tag="n")
+                nc.scalar.activation(out=n[:].rearrange("p (b y x) -> p b y x", b=NB, x=16),
+                                     in_=att[:, ob, :].rearrange("p (y b x) -> p b y x", b=NB, x=16),
+                                     func=ACT.Identity, bias=shift[:, ob:ob + 1], scale=gain[:, ob:ob + 1])
+                neg = main.tile([P, NPIX], F32, name="neg", tag="neg")
+                nc.vector.tensor_scalar(out=neg[:], in0=n[:], scalar1=0.0, scalar2=a_col[:, 0:1],
+                                        op0=ALU.min, op1=ALU.mult)
+                res = main.tile([P, NPIX], F32, name="res", tag="res")
+                nc.vector.scalar_tensor_tensor(out=res[:], in0=n[:], scalar=0.0, in1=neg[:],
+                                               op0=ALU.max, op1=ALU.add)
+                nc.sync.dma_start(out=out_v[:, ob], in_=res[:].rearrange("p (b f) -> p b f", b=NB))

@@ -20,6 +20,7 @@ BN_EPS = 1e-5
 BANK_DT = BF16
 AHEAD = 3
 T_BURST = 6
+ON_PE = ((3, 0), (2, 1), (3, 1))
 
 FLOPS = 4 * 2 * 512 * 512 * 1024
 
@@ -32,6 +33,8 @@ def tile_merge_pa_kernel(tc, x, w_c1, b_c1, w_q, w_k, w_v, bn_gamma, bn_beta, pr
 
         ident = keep.tile([P, P], F32, name="ident")
         make_identity(nc, ident[:])
+        ident_bf = keep.tile([P, P], BF16, name="ident_bf")
+        make_identity(nc, ident_bf[:])
 
         w_codes = []
         w_scales = []
@@ -54,7 +57,8 @@ def tile_merge_pa_kernel(tc, x, w_c1, b_c1, w_q, w_k, w_v, bn_gamma, bn_beta, pr
             y_scales.append(yst)
 
         att = keep.tile([P, 4, NPIX], F32, name="att")
-        stats = keep.tile([P, 4, STEPS, 6], F32, name="stats")
+        msums = keep.tile([P, 2, 4, STEPS], F32, name="msums")
+        neg_pivot = keep.tile([P, 4], F32, name="neg_pivot")
 
         bias_bf = keep.tile([P, 4], BF16, name="bias_bf")
         gam_bf = keep.tile([P, 4], BF16, name="gam_bf")
@@ -151,6 +155,16 @@ def tile_merge_pa_kernel(tc, x, w_c1, b_c1, w_q, w_k, w_v, bn_gamma, bn_beta, pr
                                      in_=s2[:].rearrange("p (j y x) -> p y x j", j=4, x=16),
                                      func=ACT.Copy, scale=0.5)
 
+            def haar_pe(b, h):
+                taps = x_sb[b][:, :, 512 * h:512 * (h + 1)].rearrange("p j (i a x e) -> p j i a x e", a=2, x=16, e=2)
+                hs = psh.tile([P, 512], F32, name="hs", tag="hs")
+                for n in range(4):
+                    nc.tensor.matmul(out=hs[:].rearrange("p (j i x) -> p j i x", j=4, x=16), lhsT=ident_bf[:],
+                                     rhs=taps[:, :, :, n // 2, :, n % 2], start=(n == 0), stop=(n == 3))
+                nc.scalar.activation(out=ll_by_image[:, b, 8 * h:8 * (h + 1)],
+                                     in_=hs[:].rearrange("p (j y x) -> p y x j", j=4, x=16),
+                                     func=ACT.Copy, scale=0.5)
+
             def prep_weight(i):
                 words = w_sb[i][:].bitcast(F32)
                 grouped = early.tile([P, 2048], BF16, name="grouped", tag="grouped", bufs=2, align_bytes=64)
@@ -165,7 +179,10 @@ def tile_merge_pa_kernel(tc, x, w_c1, b_c1, w_q, w_k, w_v, bn_gamma, bn_beta, pr
 
             prep_weight(0)
             for b in range(NB):
-                haar(b, 0)
+                if (b, 0) in ON_PE:
+                    haar_pe(b, 0)
+                else:
+                    haar(b, 0)
             quant_ll(0)
             for r in range(4):
                 bank = psh.tile([P, 4, P], BANK_DT, name="bank", tag="bank")
@@ -176,7 +193,10 @@ def tile_merge_pa_kernel(tc, x, w_c1, b_c1, w_q, w_k, w_v, bn_gamma, bn_beta, pr
             shift_copies(0)
             quant_y(0)
             for b in range(NB):
-                haar(b, 1)
+                if (b, 1) in ON_PE:
+                    haar_pe(b, 1)
+                else:
+                    haar(b, 1)
 
         with tc.tile_pool(name="main", bufs=2) as main, tc.psum_pool(name="psm", bufs=1) as psm:
             zs = {}
@@ -320,8 +340,18 @@ def tile_merge_pa_kernel(tc, x, w_c1, b_c1, w_q, w_k, w_v, bn_gamma, bn_beta, pr
                 pump_to(("G", s, 35))
                 cols = slice(P * s, P * (s + 1))
                 nc.vector.tensor_tensor(out=att[:, :, cols], in0=nums[s][:], in1=rds[s][:], op=ALU.mult)
+                if s == 0:
+                    nc.vector.tensor_scalar(out=neg_pivot[:], in0=att[:, :, 0], scalar1=-1.0, scalar2=None,
+                                            op0=ALU.mult)
+
+            def moments(s):
+                cols = slice(P * s, P * (s + 1))
                 for ob in range(4):
-                    nc.vector.bn_stats(out=stats[:, ob, s, :], in_=att[:, ob, cols])
+                    for kind, func in enumerate((ACT.Identity, ACT.Square)):
+                        junk = main.tile([P, P], F32, name="junk", tag="junk")
+                        nc.scalar.activation(out=junk[:], in_=att[:, ob, cols], func=func,
+                                             bias=neg_pivot[:, ob:ob + 1], scale=1.0,
+                                             accum_out=msums[:, kind, ob, s:s + 1])
 
             warm = main.tile([P, 1], F32, name="warm", tag="warm", bufs=1)
             with tc.manual_schedule():
@@ -345,6 +375,8 @@ def tile_merge_pa_kernel(tc, x, w_c1, b_c1, w_q, w_k, w_v, bn_gamma, bn_beta, pr
                         exps(s - 1, 0)
                     if ok(s + 1):
                         q_copy(s + 1)
+                    if ok(s - 3):
+                        moments(s - 3)
                     if ok(s - 1):
                         exps(s - 1, 1)
                     if s == 1:
@@ -355,22 +387,34 @@ def tile_merge_pa_kernel(tc, x, w_c1, b_c1, w_q, w_k, w_v, bn_gamma, bn_beta, pr
                         one_over_den(s - 2)
                 divide(STEPS - 3)
                 exps(STEPS - 1, 0)
+                moments(STEPS - 3)
                 weigh(STEPS - 2, 0, 9)
                 one_over_den(STEPS - 2)
                 exps(STEPS - 1, 1)
                 exps(STEPS - 1, 2)
                 weigh(STEPS - 1, 0, 6)
                 divide(STEPS - 2)
+                moments(STEPS - 2)
                 weigh(STEPS - 1, 6, 9)
                 one_over_den(STEPS - 1)
                 nc.scalar.activation(out=warm[:], in_=rds[STEPS - 1][:, 0, 0:1], func=ACT.Sqrt)
                 divide(STEPS - 1)
+                moments(STEPS - 1)
 
-            mv = main.tile([P, 4, 2], F32, name="mv", tag="mv", bufs=1)
-            for ob in range(4):
-                nc.vector.bn_aggr(out=mv[:, ob, :], in_=stats[:, ob, :, :].rearrange("p s k -> p (s k)"))
+            tot = main.tile([P, 2, 4], F32, name="tot", tag="tot", bufs=1)
+            nc.vector.tensor_reduce(out=tot[:].rearrange("p k o -> p (k o)"),
+                                    in_=msums[:].rearrange("p k o s -> p (k o) s"),
+                                    axis=mybir.AxisListType.X, op=ALU.add)
+            avg = main.tile([P, 2, 4], F32, name="avg", tag="avg", bufs=1)
+            nc.vector.tensor_scalar(out=avg[:], in0=tot[:], scalar1=1.0 / NPIX, scalar2=None, op0=ALU.mult)
+            dd = main.tile([P, 4], F32, name="dd", tag="dd", bufs=1)
+            nc.vector.tensor_tensor(out=dd[:], in0=avg[:, 0, :], in1=avg[:, 0, :], op=ALU.mult)
+            var = main.tile([P, 4], F32, name="var", tag="var", bufs=1)
+            nc.vector.tensor_tensor(out=var[:], in0=avg[:, 1, :], in1=dd[:], op=ALU.subtract)
             ve = main.tile([P, 4], F32, name="ve", tag="ve", bufs=1)
-            nc.vector.tensor_scalar(out=ve[:], in0=mv[:, :, 1], scalar1=BN_EPS, scalar2=None, op0=ALU.add)
+            nc.vector.tensor_scalar(out=ve[:], in0=var[:], scalar1=BN_EPS, scalar2=None, op0=ALU.add)
+            mean = main.tile([P, 4], F32, name="mean", tag="mean", bufs=1)
+            nc.vector.tensor_tensor(out=mean[:], in0=avg[:, 0, :], in1=neg_pivot[:], op=ALU.subtract)
             sd = main.tile([P, 4], F32, name="sd", tag="sd", bufs=1)
             nc.scalar.activation(out=sd[:], in_=ve[:], func=ACT.Sqrt)
             rstd = main.tile([P, 4], F32, name="rstd", tag="rstd", bufs=1)
@@ -378,7 +422,7 @@ def tile_merge_pa_kernel(tc, x, w_c1, b_c1, w_q, w_k, w_v, bn_gamma, bn_beta, pr
             gain = main.tile([P, 4], F32, name="gain", tag="gain", bufs=1)
             nc.vector.tensor_tensor(out=gain[:], in0=gam_bf[:], in1=rstd[:], op=ALU.mult)
             mg = main.tile([P, 4], F32, name="mg", tag="mg", bufs=1)
-            nc.vector.tensor_tensor(out=mg[:], in0=mv[:, :, 0], in1=gain[:], op=ALU.mult)
+            nc.vector.tensor_tensor(out=mg[:], in0=mean[:], in1=gain[:], op=ALU.mult)
             shift = main.tile([P, 4], F32, name="shift", tag="shift", bufs=1)
             nc.vector.tensor_tensor(out=shift[:], in0=bet_bf[:], in1=mg[:], op=ALU.subtract)
             out_v = out.rearrange("b (c r) h w -> c r b (h w)", r=4)

@@ -20,7 +20,10 @@ BN_EPS = 1e-5
 BANK_DT = BF16
 AHEAD = 3
 T_BURST = 6
-ON_PE = ((3, 0), (2, 1), (3, 1))
+LAST_ON_VECTOR = 3
+PIECES = ((0, 4), (4, 4), (8, 8))
+HAAR_ON_VECTOR = ((1, 2), (1, 3), (2, 0), (2, 1), (2, 2), (2, 3))
+W_C1, W_K, W_Q, W_V = 0, 1, 2, 3
 
 FLOPS = 4 * 2 * 512 * 512 * 1024
 
@@ -30,11 +33,48 @@ def tile_merge_pa_kernel(tc, x, w_c1, b_c1, w_q, w_k, w_v, bn_gamma, bn_beta, pr
     with ExitStack() as ctx:
         keep = ctx.enter_context(tc.tile_pool(name="keep", bufs=1))
         mid = ctx.enter_context(tc.tile_pool(name="mid", bufs=1))
+        main = ctx.enter_context(tc.tile_pool(name="main", bufs=2))
+        psm = ctx.enter_context(tc.psum_pool(name="psm", bufs=1))
+        ctx.enter_context(tc.manual_schedule())
+
+        weights = (w_c1, w_k, w_q, w_v)
+        w_all = main.tile([P, 4, 4, 512], BF16, name="w_all", tag="z", bufs=3)
+        x_ab = main.tile([P, 2, NB, 4, 256], BF16, name="x_ab", tag="ev", bufs=2)
+        x_c = main.tile([P, NB, 4, 512], BF16, name="x_c", tag="ev", bufs=2)
+
+        def x_piece(pc, b):
+            return x_c[:, b] if pc == 2 else x_ab[:, pc, b]
+
+        def load_w(i):
+            nc.sync.dma_start(out=w_all[:, i], in_=weights[i].rearrange("(c r) k -> c r k", r=4))
+
+        def load_x(pc):
+            row0, nr = PIECES[pc]
+            for b in range(NB):
+                nc.sync.dma_start(out=x_piece(pc, b),
+                                  in_=x[b].rearrange("(p j) h w -> p j (h w)", j=4)[:, :, ROW * row0:ROW * (row0 + nr)])
+
+        bias_bf = keep.tile([P, 4], BF16, name="bias_bf")
+        nc.sync.dma_start(out=bias_bf[:], in_=b_c1.rearrange("(p t) -> p t", t=4))
+        load_w(W_C1)
+        load_x(0)
+        load_w(W_Q)
+        load_w(W_K)
+        load_x(1)
+        load_w(W_V)
+        load_x(2)
 
         ident = keep.tile([P, P], F32, name="ident")
         make_identity(nc, ident[:])
         ident_bf = keep.tile([P, P], BF16, name="ident_bf")
         make_identity(nc, ident_bf[:])
+
+        gam_bf = keep.tile([P, 4], BF16, name="gam_bf")
+        bet_bf = keep.tile([P, 4], BF16, name="bet_bf")
+        a_bf = keep.tile([P, 1], BF16, name="a_bf")
+
+        warm = keep.tile([P, 1], F32, name="warm")
+        nc.scalar.activation(out=warm[:], in_=ident[:, 0:1], func=ACT.Exp)
 
         w_codes = []
         w_scales = []
@@ -59,382 +99,417 @@ def tile_merge_pa_kernel(tc, x, w_c1, b_c1, w_q, w_k, w_v, bn_gamma, bn_beta, pr
         att = keep.tile([P, 4, NPIX], F32, name="att")
         msums = keep.tile([P, 2, 4, STEPS], F32, name="msums")
         neg_pivot = keep.tile([P, 4], F32, name="neg_pivot")
-
-        bias_bf = keep.tile([P, 4], BF16, name="bias_bf")
-        gam_bf = keep.tile([P, 4], BF16, name="gam_bf")
-        bet_bf = keep.tile([P, 4], BF16, name="bet_bf")
-        a_bf = keep.tile([P, 1], BF16, name="a_bf")
-        nc.gpsimd.dma_start(out=bias_bf[:], in_=b_c1.rearrange("(p t) -> p t", t=4))
-        nc.gpsimd.dma_start(out=gam_bf[:], in_=bn_gamma.rearrange("(p t) -> p t", t=4))
-        nc.gpsimd.dma_start(out=bet_bf[:], in_=bn_beta.rearrange("(p t) -> p t", t=4))
-        nc.gpsimd.dma_start(out=a_bf[:], in_=prelu_a.partition_broadcast(P))
         a_col = keep.tile([P, 1], F32, name="a_col")
-        nc.vector.tensor_copy(out=a_col[:], in_=a_bf[:])
         zeros_bf = keep.tile([P, P], BF16, name="zeros_bf")
-        nc.vector.memset(zeros_bf[:], 0.0)
         bias_full = keep.tile([P, P, 4], BF16, name="bias_full")
-        for t in range(4):
-            nc.vector.tensor_scalar(out=bias_full[:, :, t], in0=zeros_bf[:], scalar1=bias_bf[:, t:t + 1],
-                                    scalar2=None, op0=ALU.add)
 
         ll = mid.tile([P, NPIX, 4], BF16, name="ll", align_bytes=64)
         y_mid = mid.tile([P, NPIX, 4], BF16, name="y_mid", align_bytes=64)
         y_left = mid.tile([P, NPIX, 4], BF16, name="y_left", align_bytes=64)
         y_right = mid.tile([P, NPIX, 4], BF16, name="y_right", align_bytes=64)
-        nc.gpsimd.memset(y_left[:], 0.0)
-        nc.gpsimd.memset(y_right[:], 0.0)
         ll_by_image = ll[:].rearrange("p (y b x) j -> p b y x j", b=NB, x=16)
         ll_flat = ll[:].rearrange("p c j -> p (c j)")
         lefts = y_left[:].rearrange("p (g x) t -> p g (x t)", x=16)
         mids = y_mid[:].rearrange("p (g x) t -> p g (x t)", x=16)
         rights = y_right[:].rearrange("p (g x) t -> p g (x t)", x=16)
+        nc.gpsimd.memset(lefts[:, :, 0:8], 0.0)
+        nc.gpsimd.memset(rights[:, :, 56:64], 0.0)
+        nc.gpsimd.dma_start(out=gam_bf[:], in_=bn_gamma.rearrange("(p t) -> p t", t=4))
+        nc.gpsimd.dma_start(out=bet_bf[:], in_=bn_beta.rearrange("(p t) -> p t", t=4))
+        nc.gpsimd.dma_start(out=a_bf[:], in_=prelu_a.partition_broadcast(P))
 
-        def quant_ll(h):
-            nc.vector.quantize_mx(out=ll_codes[:, 512 * h:512 * (h + 1)].bitcast(FP8X4),
-                                  scales=ll_scales[:, 512 * h:512 * (h + 1)],
-                                  in_=ll_flat[:, 2048 * h:2048 * (h + 1)])
+        zs = {}
+        evs = {}
+        nums = {}
+        dens = {}
+        q_sbs = {}
+        rds = {}
+        lgs = {}
+        banks = {}
+
+        def ok(s):
+            return 0 <= s < STEPS
+
+        def conv(dst, s, j, wi):
+            c0 = ROW + P * s + ROW * (j // 3 - 1)
+            d = j % 3
+            nc.tensor.matmul_mx(out=dst, lhsT=y_codes[d][:, c0:c0 + P].bitcast(FP8X4),
+                                lhsT_scale=y_scales[d][:, c0:c0 + P],
+                                rhs=w_codes[wi][:].bitcast(FP8X4), rhs_scale=w_scales[wi][:],
+                                start=True, stop=True)
 
         def first_conv(bank, r):
             cols = slice(P * r, P * (r + 1))
             for t in range(4):
                 nc.tensor.matmul_mx(out=bank[:, t, :],
-                                    lhsT=w_codes[0][:, P * t:P * (t + 1)].bitcast(FP8X4),
-                                    lhsT_scale=w_scales[0][:, P * t:P * (t + 1)],
+                                    lhsT=w_codes[W_C1][:, P * t:P * (t + 1)].bitcast(FP8X4),
+                                    lhsT_scale=w_scales[W_C1][:, P * t:P * (t + 1)],
                                     rhs=ll_codes[:, cols].bitcast(FP8X4), rhs_scale=ll_scales[:, cols],
                                     start=True, stop=True)
 
-        def add_bias(bank, r):
-            nc.vector.tensor_tensor(out=y_mid[:, P * r:P * (r + 1), :], in0=bank[:].rearrange("p t n -> p n t"),
+        def add_up(dst, src, i):
+            ob = i // 9
+            j = i % 9
+            nc.tensor.matmul(out=dst[:, ob, :], lhsT=src[:, j, P * ob:P * (ob + 1)], rhs=ident[:],
+                             is_transpose=True, start=(j == 0), stop=(j == 8))
+
+        def emit_pe(tok):
+            kind, s, j = tok
+            if kind == "q":
+                q_ps = psm.tile([P, 512], F32, name="q_ps", tag="k_ps", bufs=3)
+                conv(q_ps[:], s, 4, W_Q)
+                banks[tok] = q_ps
+            elif kind == "k":
+                k_ps = psm.tile([P, 512], F32, name="k_ps", tag="k_ps", bufs=3)
+                conv(k_ps[:], s, j, W_K)
+                banks[tok] = k_ps
+            elif kind == "v":
+                v_ps = psm.tile([P, 512], F32, name="v_ps", tag="v_ps", bufs=3)
+                conv(v_ps[:], s, j, W_V)
+                banks[tok] = v_ps
+            elif kind == "c":
+                bank = psm.tile([P, 4, P], BANK_DT, name="bank", tag="v_ps", bufs=3)
+                first_conv(bank, s)
+                banks[tok] = bank
+            elif kind == "w":
+                words = w_all[:, s].bitcast(F32)
+                wT = psm.tile([P, 2, 2, P], F32, name="wT", tag=("k_ps" if s != W_V else "v_ps"), bufs=3)
+                for rr in range(2):
+                    for u in range(2):
+                        nc.tensor.transpose(wT[:, rr, u, :], words[:, 2 * j + rr, u:256:2], ident[:])
+                banks[tok] = wT
+            elif kind == "h":
+                nr = PIECES[s][1]
+                taps = x_piece(s, j).rearrange("p j (i a x e) -> p j i a x e", a=2, x=16, e=2)
+                if j == NB - 1:
+                    hs = psm.tile([P, 512], F32, name="hs_last", tag="den", bufs=1)
+                else:
+                    hs = psm.tile([P, 512], F32, name="hs", tag="v_ps", bufs=3)
+                for n in range(4):
+                    nc.tensor.matmul(out=hs[:, 0:ROW * nr].rearrange("p (j i x) -> p j i x", j=4, x=16), lhsT=ident_bf[:],
+                                     rhs=taps[:, :, :, n // 2, :, n % 2], start=(n == 0), stop=(n == 3))
+                banks[tok] = hs
+            elif kind == "F":
+                if j == 0:
+                    if s == STEPS - 1:
+                        den = psm.tile([P, 4, P], F32, name="den_last", tag="k_ps", bufs=3)
+                    else:
+                        den = psm.tile([P, 4, P], F32, name="den", tag="den", bufs=1)
+                    dens[s] = den
+                add_up(dens[s], zs[s], j)
+            else:
+                if j == 0:
+                    if s == STEPS - 1:
+                        num = psm.tile([P, 4, P], F32, name="num_last", tag="k_ps", bufs=3)
+                    else:
+                        num = psm.tile([P, 4, P], F32, name="num", tag="num", bufs=1)
+                    nums[s] = num
+                add_up(nums[s], evs[s], j)
+
+        def on_pe(pc):
+            return [("h", pc, b) for b in range(NB) if (pc, b) not in HAAR_ON_VECTOR]
+
+        pe_list = [("w", W_C1, 0), ("w", W_C1, 1)] + on_pe(0) + [("w", W_Q, 0), ("w", W_Q, 1), ("c", 0, 0), ("c", 1, 0),
+                                                                 ("w", W_K, 0), ("w", W_K, 1)] + on_pe(1)
+        pe_list += [("q", 0, 0)] + [("k", 0, j) for j in range(AHEAD)]
+        for s in range(STEPS + 2):
+            mms = []
+            if ok(s):
+                mms.extend([("k", s, j) for j in range(AHEAD, 9)])
+            if ok(s + 1):
+                mms.append(("q", s + 1, 0))
+            if s == 0:
+                mms.extend([("c", 2, 0), ("c", 3, 0), ("w", W_V, 0), ("w", W_V, 1)] + on_pe(2))
+            if s == 1:
+                mms.extend([("c", r, 0) for r in range(4, 8)])
+            sums = []
+            if ok(s - 2):
+                mms.extend([("v", s - 2, j) for j in range(AHEAD, 9)])
+                sums = [("F", s - 2, i) for i in range(36)]
+            if s == STEPS:
+                pe_list.extend(sums)
+                sums = []
+            for n, tok in enumerate(mms):
+                pe_list.append(tok)
+                if n % 2 == 1:
+                    pe_list.extend(sums[:T_BURST])
+                    sums = sums[T_BURST:]
+            pe_list.extend(sums)
+            if ok(s + 1):
+                pe_list.extend([("k", s + 1, j) for j in range(AHEAD)])
+            if ok(s - 1):
+                pe_list.extend([("v", s - 1, j) for j in range(AHEAD)])
+            if ok(s - 2):
+                pe_list.extend([("G", s - 2, i) for i in range(36)])
+
+        done = set()
+        pos = [0]
+
+        def pump_to(tok):
+            while tok not in done:
+                nxt = pe_list[pos[0]]
+                pos[0] += 1
+                emit_pe(nxt)
+                done.add(nxt)
+
+        def weight_copies(i):
+            grouped = main.tile([P, 2048], BF16, name="grouped", tag="grouped", bufs=2, align_bytes=64)
+            gwords = grouped[:].bitcast(F32).rearrange("p (r c u) -> p r c u", r=4, u=2)
+            for h in range(2):
+                pump_to(("w", i, h))
+                nc.scalar.copy(out=gwords[:, 2 * h:2 * h + 2], in_=banks[("w", i, h)][:].rearrange("p r u c -> p r c u"))
+            return grouped
+
+        def quant_w(i, grouped):
+            nc.vector.quantize_mx(out=w_codes[i][:].bitcast(FP8X4), scales=w_scales[i][:], in_=grouped[:])
+
+        def halve(pc, b, sums):
+            row0, nr = PIECES[pc]
+            nc.scalar.activation(out=ll_by_image[:, b, row0:row0 + nr],
+                                 in_=sums.rearrange("p (j y x) -> p y x j", j=4, x=16),
+                                 func=ACT.Copy, scale=0.5)
+
+        def haar_from_pe(pc):
+            for tok in on_pe(pc):
+                pump_to(tok)
+                halve(pc, tok[2], banks[tok][:, 0:ROW * PIECES[pc][1]])
+
+        def haar_on_vector(pc, b):
+            nr = PIECES[pc][1]
+            rows = x_piece(pc, b).rearrange("p j (i a w) -> p j i a w", a=2, w=32)
+            s1 = main.tile([P, 4, nr, 32], F32, name="s1", tag="s1", bufs=2)
+            nc.vector.tensor_tensor(out=s1[:], in0=rows[:, :, :, 0, :], in1=rows[:, :, :, 1, :], op=ALU.add)
+            pairs = s1[:].rearrange("p j i (x e) -> p (j i x) e", e=2)
+            s2 = main.tile([P, ROW * nr], F32, name="s2", tag="s2", bufs=2)
+            nc.vector.tensor_tensor(out=s2[:], in0=pairs[:, :, 0], in1=pairs[:, :, 1], op=ALU.add)
+            halve(pc, b, s2[:])
+
+        def quant_ll(pc):
+            c0 = ROW * PIECES[pc][0]
+            n = ROW * PIECES[pc][1]
+            nc.vector.quantize_mx(out=ll_codes[:, c0:c0 + n].bitcast(FP8X4), scales=ll_scales[:, c0:c0 + n],
+                                  in_=ll_flat[:, 4 * c0:4 * (c0 + n)])
+
+        def add_bias(r):
+            pump_to(("c", r, 0))
+            nc.vector.tensor_tensor(out=y_mid[:, P * r:P * (r + 1), :], in0=banks[("c", r, 0)][:].rearrange("p t n -> p n t"),
                                     in1=bias_full[:], op=ALU.add)
 
-        def shift_copies(h):
-            g0 = 32 * h
-            nc.scalar.copy(out=lefts[:, g0:g0 + 32, 4:64], in_=mids[:, g0:g0 + 32, 0:60])
-            nc.scalar.copy(out=rights[:, g0:g0 + 32, 0:60], in_=mids[:, g0:g0 + 32, 4:64])
+        def shift_copies(pc, on_vector):
+            g0 = NB * PIECES[pc][0]
+            g1 = g0 + NB * PIECES[pc][1]
+            if on_vector:
+                nc.vector.tensor_copy(out=lefts[:, g0:g1, 4:64], in_=mids[:, g0:g1, 0:60])
+                nc.vector.tensor_copy(out=rights[:, g0:g1, 0:60], in_=mids[:, g0:g1, 4:64])
+            else:
+                nc.scalar.copy(out=lefts[:, g0:g1, 4:64], in_=mids[:, g0:g1, 0:60])
+                nc.scalar.copy(out=rights[:, g0:g1, 0:60], in_=mids[:, g0:g1, 4:64])
 
-        def quant_y(h):
-            c0 = ROW + 512 * h
-            for d, ysrc in enumerate((y_left, y_mid, y_right)):
-                nc.vector.quantize_mx(out=y_codes[d][:, c0:c0 + 512].bitcast(FP8X4),
-                                      scales=y_scales[d][:, c0:c0 + 512],
-                                      in_=ysrc[:].rearrange("p c j -> p (c j)")[:, 2048 * h:2048 * (h + 1)])
+        def quant_y(pc):
+            p0 = ROW * PIECES[pc][0]
+            n = ROW * PIECES[pc][1]
+            for d, ysrc in ((1, y_mid), (0, y_left), (2, y_right)):
+                nc.vector.quantize_mx(out=y_codes[d][:, ROW + p0:ROW + p0 + n].bitcast(FP8X4),
+                                      scales=y_scales[d][:, ROW + p0:ROW + p0 + n],
+                                      in_=ysrc[:].rearrange("p c j -> p (c j)")[:, 4 * p0:4 * (p0 + n)])
 
-        with tc.tile_pool(name="early", bufs=1) as early, tc.psum_pool(name="psh", bufs=2) as psh:
-            weights = (w_c1, w_k, w_q, w_v)
-            x_sb = []
-            w_sb = []
-            for i in range(4):
-                xt = early.tile([P, 4, 1024], BF16, name="x_sb%d" % i)
-                x_sb.append(xt)
-                wt = early.tile([P, 4, 512], BF16, name="w_sb%d" % i)
-                w_sb.append(wt)
+        def q_copy(s):
+            pump_to(("q", s, 0))
+            q_sb = main.tile([P, 512], F32, name="q_sb", tag="q_sb")
+            nc.scalar.copy(out=q_sb[:], in_=banks[("q", s, 0)][:])
+            q_sbs[s] = q_sb
 
-            def load_w(i):
-                nc.sync.dma_start(out=w_sb[i][:], in_=weights[i].rearrange("(c r) k -> c r k", r=4))
+        def scores(s):
+            z = main.tile([P, 9, 512], F32, name="z", tag="z", bufs=3)
+            zs[s] = z
+            for j in range(9):
+                pump_to(("k", s, j))
+                nc.vector.tensor_tensor(out=z[:, j, :], in0=q_sbs[s][:], in1=banks[("k", s, j)][:], op=ALU.mult)
 
-            def load_x(b, h):
-                nc.sync.dma_start(out=x_sb[b][:, :, 512 * h:512 * (h + 1)],
-                                  in_=x[b].rearrange("(p j) h w -> p j (h w)", j=4)[:, :, 512 * h:512 * (h + 1)])
+        def shift_by_max(s, on_vector=0):
+            z = zs[s]
+            t1 = main.tile([P, 4, 512], F32, name="t1", tag="t1", bufs=1)
+            nc.vector.tensor_tensor(out=t1[:], in0=z[:, 0:4, :], in1=z[:, 4:8, :], op=ALU.max)
+            t2 = main.tile([P, 2, 512], F32, name="t2", tag="t2", bufs=1)
+            nc.vector.tensor_tensor(out=t2[:], in0=t1[:, 0:2, :], in1=t1[:, 2:4, :], op=ALU.max)
+            t3 = main.tile([P, 512], F32, name="t3", tag="t3", bufs=1)
+            nc.vector.tensor_tensor(out=t3[:], in0=t2[:, 0, :], in1=t2[:, 1, :], op=ALU.max)
+            m = main.tile([P, 512], F32, name="m", tag="m")
+            nc.vector.tensor_tensor(out=m[:], in0=t3[:], in1=z[:, 8, :], op=ALU.max)
+            for j in range(on_vector):
+                nc.vector.tensor_tensor(out=z[:, j, :], in0=z[:, j, :], in1=m[:], op=ALU.subtract)
+            for j in range(on_vector, 9):
+                nc.gpsimd.tensor_tensor(out=z[:, j, :], in0=z[:, j, :], in1=m[:], op=ALU.subtract)
 
-            load_w(0)
-            for b in range(NB):
-                load_x(b, 0)
-            for i in range(1, 4):
-                load_w(i)
-            for b in range(NB):
-                load_x(b, 1)
+        def exps(s, g):
+            z = zs[s]
+            nc.scalar.activation(out=z[:, 3 * g:3 * g + 3, :], in_=z[:, 3 * g:3 * g + 3, :], func=ACT.Exp)
 
-            def haar(b, h):
-                rows = x_sb[b][:, :, 512 * h:512 * (h + 1)].rearrange("p j (i a w) -> p j i a w", a=2, w=32)
-                s1 = early.tile([P, 4, 8, 32], F32, name="s1", tag="s1", bufs=2)
-                nc.vector.tensor_tensor(out=s1[:], in0=rows[:, :, :, 0, :], in1=rows[:, :, :, 1, :], op=ALU.add)
-                pairs = s1[:].rearrange("p j i (x e) -> p (j i x) e", e=2)
-                s2 = early.tile([P, 512], F32, name="s2", tag="s2", bufs=2)
-                nc.vector.tensor_tensor(out=s2[:], in0=pairs[:, :, 0], in1=pairs[:, :, 1], op=ALU.add)
-                nc.scalar.activation(out=ll_by_image[:, b, 8 * h:8 * (h + 1)],
-                                     in_=s2[:].rearrange("p (j y x) -> p y x j", j=4, x=16),
-                                     func=ACT.Copy, scale=0.5)
+        def weigh(s, j0, j1):
+            if j0 == 0:
+                ev = main.tile([P, 9, 512], F32, name="ev", tag="ev", bufs=2)
+                evs[s] = ev
+            for j in range(j0, j1):
+                pump_to(("v", s, j))
+                nc.vector.tensor_tensor(out=evs[s][:, j, :], in0=zs[s][:, j, :], in1=banks[("v", s, j)][:],
+                                        op=ALU.mult)
 
-            def haar_pe(b, h):
-                taps = x_sb[b][:, :, 512 * h:512 * (h + 1)].rearrange("p j (i a x e) -> p j i a x e", a=2, x=16, e=2)
-                hs = psh.tile([P, 512], F32, name="hs", tag="hs")
-                for n in range(4):
-                    nc.tensor.matmul(out=hs[:].rearrange("p (j i x) -> p j i x", j=4, x=16), lhsT=ident_bf[:],
-                                     rhs=taps[:, :, :, n // 2, :, n % 2], start=(n == 0), stop=(n == 3))
-                nc.scalar.activation(out=ll_by_image[:, b, 8 * h:8 * (h + 1)],
-                                     in_=hs[:].rearrange("p (j y x) -> p y x j", j=4, x=16),
-                                     func=ACT.Copy, scale=0.5)
+        def log_den(s):
+            pump_to(("F", s, 35))
+            lg = main.tile([P, 4, P], F32, name="lg", tag="lg")
+            nc.scalar.activation(out=lg[:], in_=dens[s][:], func=ACT.Ln)
+            lgs[s] = lg
 
-            def prep_weight(i):
-                words = w_sb[i][:].bitcast(F32)
-                grouped = early.tile([P, 2048], BF16, name="grouped", tag="grouped", bufs=2, align_bytes=64)
-                gwords = grouped[:].bitcast(F32).rearrange("p (r c u) -> p r c u", r=4, u=2)
-                for h in range(2):
-                    wT = psh.tile([P, 2, 2, P], F32, name="wT", tag="wT")
-                    for rr in range(2):
-                        for u in range(2):
-                            nc.tensor.transpose(wT[:, rr, u, :], words[:, 2 * h + rr, u:256:2], ident[:])
-                    nc.scalar.copy(out=gwords[:, 2 * h:2 * h + 2], in_=wT[:].rearrange("p r u c -> p r c u"))
-                nc.vector.quantize_mx(out=w_codes[i][:].bitcast(FP8X4), scales=w_scales[i][:], in_=grouped[:])
+        def exp_minus_log(s):
+            rd = main.tile([P, 4, P], F32, name="rd", tag="rd")
+            nc.scalar.activation(out=rd[:], in_=lgs[s][:], func=ACT.Exp, scale=-1.0)
+            rds[s] = rd
 
-            prep_weight(0)
-            for b in range(NB):
-                if (b, 0) in ON_PE:
-                    haar_pe(b, 0)
-                else:
-                    haar(b, 0)
-            quant_ll(0)
-            for r in range(4):
-                bank = psh.tile([P, 4, P], BANK_DT, name="bank", tag="bank")
-                first_conv(bank, r)
-                add_bias(bank, r)
-            for i in range(1, 4):
-                prep_weight(i)
-            shift_copies(0)
-            quant_y(0)
-            for b in range(NB):
-                if (b, 1) in ON_PE:
-                    haar_pe(b, 1)
-                else:
-                    haar(b, 1)
+        def one_over_den(s):
+            log_den(s)
+            exp_minus_log(s)
 
-        with tc.tile_pool(name="main", bufs=2) as main, tc.psum_pool(name="psm", bufs=1) as psm:
-            zs = {}
-            evs = {}
-            nums = {}
-            dens = {}
-            q_sbs = {}
-            rds = {}
-            banks = {}
+        def divide(s):
+            pump_to(("G", s, 35))
+            cols = slice(P * s, P * (s + 1))
+            nc.vector.tensor_tensor(out=att[:, :, cols], in0=nums[s][:], in1=rds[s][:], op=ALU.mult)
+            if s == 0:
+                nc.vector.tensor_scalar(out=neg_pivot[:], in0=att[:, :, 0], scalar1=-1.0, scalar2=None,
+                                        op0=ALU.mult)
 
-            def ok(s):
-                return 0 <= s < STEPS
-
-            def conv(dst, s, j, wi):
-                c0 = ROW + P * s + ROW * (j // 3 - 1)
-                d = j % 3
-                nc.tensor.matmul_mx(out=dst, lhsT=y_codes[d][:, c0:c0 + P].bitcast(FP8X4),
-                                    lhsT_scale=y_scales[d][:, c0:c0 + P],
-                                    rhs=w_codes[wi][:].bitcast(FP8X4), rhs_scale=w_scales[wi][:],
-                                    start=True, stop=True)
-
-            pe_list = [("q", 0, 0)] + [("k", 0, j) for j in range(AHEAD)]
-            for s in range(STEPS + 2):
-                mms = []
-                if ok(s):
-                    mms.extend([("k", s, j) for j in range(AHEAD, 9)])
-                if ok(s + 1):
-                    mms.append(("q", s + 1, 0))
-                if s == 1:
-                    mms.extend([("c", r, 0) for r in range(4, 8)])
-                sums = []
-                if ok(s - 2):
-                    mms.extend([("v", s - 2, j) for j in range(AHEAD, 9)])
-                    sums = [("F", s - 2, i) for i in range(36)]
-                for n, tok in enumerate(mms):
-                    pe_list.append(tok)
-                    if n % 2 == 1:
-                        pe_list.extend(sums[:T_BURST])
-                        sums = sums[T_BURST:]
-                pe_list.extend(sums)
-                if ok(s + 1):
-                    pe_list.extend([("k", s + 1, j) for j in range(AHEAD)])
-                if ok(s - 1):
-                    pe_list.extend([("v", s - 1, j) for j in range(AHEAD)])
-                if ok(s - 2):
-                    pe_list.extend([("G", s - 2, i) for i in range(36)])
-
-            def add_up(dst, src, i):
-                ob = i // 9
-                j = i % 9
-                nc.tensor.matmul(out=dst[:, ob, :], lhsT=src[:, j, P * ob:P * (ob + 1)], rhs=ident[:],
-                                 is_transpose=True, start=(j == 0), stop=(j == 8))
-
-            def emit_pe(tok):
-                kind, s, j = tok
-                if kind == "q":
-                    q_ps = psm.tile([P, 512], F32, name="q_ps", tag="k_ps", bufs=3)
-                    conv(q_ps[:], s, 4, 2)
-                    banks[tok] = q_ps
-                elif kind == "k":
-                    k_ps = psm.tile([P, 512], F32, name="k_ps", tag="k_ps", bufs=3)
-                    conv(k_ps[:], s, j, 1)
-                    banks[tok] = k_ps
-                elif kind == "v":
-                    v_ps = psm.tile([P, 512], F32, name="v_ps", tag="v_ps", bufs=3)
-                    conv(v_ps[:], s, j, 3)
-                    banks[tok] = v_ps
-                elif kind == "c":
-                    bank2 = psm.tile([P, 4, P], BANK_DT, name="bank2", tag="v_ps", bufs=3)
-                    first_conv(bank2, s)
-                    banks[tok] = bank2
-                elif kind == "F":
-                    if j == 0:
-                        den = psm.tile([P, 4, P], F32, name="den", tag="den", bufs=1)
-                        dens[s] = den
-                    add_up(dens[s], zs[s], j)
-                else:
-                    if j == 0:
-                        num = psm.tile([P, 4, P], F32, name="num", tag="num", bufs=1)
-                        nums[s] = num
-                    add_up(nums[s], evs[s], j)
-
-            done = set()
-            pos = [0]
-
-            def pump_to(tok):
-                while tok not in done:
-                    nxt = pe_list[pos[0]]
-                    pos[0] += 1
-                    emit_pe(nxt)
-                    done.add(nxt)
-
-            def q_copy(s):
-                pump_to(("q", s, 0))
-                q_sb = main.tile([P, 512], F32, name="q_sb", tag="q_sb")
-                nc.scalar.copy(out=q_sb[:], in_=banks[("q", s, 0)][:])
-                q_sbs[s] = q_sb
-
-            def scores(s):
-                z = main.tile([P, 9, 512], F32, name="z", tag="z", bufs=3)
-                zs[s] = z
-                for j in range(9):
-                    pump_to(("k", s, j))
-                    nc.vector.tensor_tensor(out=z[:, j, :], in0=q_sbs[s][:], in1=banks[("k", s, j)][:], op=ALU.mult)
-
-            def shift_by_max(s):
-                z = zs[s]
-                t1 = main.tile([P, 4, 512], F32, name="t1", tag="t1", bufs=1)
-                nc.vector.tensor_tensor(out=t1[:], in0=z[:, 0:4, :], in1=z[:, 4:8, :], op=ALU.max)
-                t2 = main.tile([P, 2, 512], F32, name="t2", tag="t2", bufs=1)
-                nc.vector.tensor_tensor(out=t2[:], in0=t1[:, 0:2, :], in1=t1[:, 2:4, :], op=ALU.max)
-                t3 = main.tile([P, 512], F32, name="t3", tag="t3", bufs=1)
-                nc.vector.tensor_tensor(out=t3[:], in0=t2[:, 0, :], in1=t2[:, 1, :], op=ALU.max)
-                m = main.tile([P, 512], F32, name="m", tag="m")
-                nc.vector.tensor_tensor(out=m[:], in0=t3[:], in1=z[:, 8, :], op=ALU.max)
-                for j in range(9):
-                    nc.gpsimd.tensor_tensor(out=z[:, j, :], in0=z[:, j, :], in1=m[:], op=ALU.subtract)
-
-            def exps(s, g):
-                z = zs[s]
-                nc.scalar.activation(out=z[:, 3 * g:3 * g + 3, :], in_=z[:, 3 * g:3 * g + 3, :], func=ACT.Exp)
-
-            def weigh(s, j0, j1):
-                if j0 == 0:
-                    ev = main.tile([P, 9, 512], F32, name="ev", tag="ev", bufs=2)
-                    evs[s] = ev
-                for j in range(j0, j1):
-                    pump_to(("v", s, j))
-                    nc.vector.tensor_tensor(out=evs[s][:, j, :], in0=zs[s][:, j, :], in1=banks[("v", s, j)][:],
-                                            op=ALU.mult)
-
-            def one_over_den(s):
-                pump_to(("F", s, 35))
-                lg = main.tile([P, 4, P], F32, name="lg", tag="lg")
-                nc.scalar.activation(out=lg[:], in_=dens[s][:], func=ACT.Ln)
-                rd = main.tile([P, 4, P], F32, name="rd", tag="rd")
-                nc.scalar.activation(out=rd[:], in_=lg[:], func=ACT.Exp, scale=-1.0)
-                rds[s] = rd
-
-            def divide(s):
-                pump_to(("G", s, 35))
-                cols = slice(P * s, P * (s + 1))
-                nc.vector.tensor_tensor(out=att[:, :, cols], in0=nums[s][:], in1=rds[s][:], op=ALU.mult)
-                if s == 0:
-                    nc.vector.tensor_scalar(out=neg_pivot[:], in0=att[:, :, 0], scalar1=-1.0, scalar2=None,
-                                            op0=ALU.mult)
-
-            def moments(s):
-                cols = slice(P * s, P * (s + 1))
-                for ob in range(4):
-                    for kind, func in enumerate((ACT.Identity, ACT.Square)):
-                        junk = main.tile([P, P], F32, name="junk", tag="junk")
-                        nc.scalar.activation(out=junk[:], in_=att[:, ob, cols], func=func,
-                                             bias=neg_pivot[:, ob:ob + 1], scale=1.0,
-                                             accum_out=msums[:, kind, ob, s:s + 1])
-
-            warm = main.tile([P, 1], F32, name="warm", tag="warm", bufs=1)
-            with tc.manual_schedule():
-                q_copy(0)
-                for s in range(STEPS):
-                    scores(s)
-                    if s == 1:
-                        for r in range(4, 8):
-                            pump_to(("c", r, 0))
-                            add_bias(banks[("c", r, 0)], r)
-                    if s == 2:
-                        quant_y(1)
-                    if ok(s - 3):
-                        divide(s - 3)
-                    if ok(s - 2):
-                        weigh(s - 2, 0, 9)
-                    shift_by_max(s)
-                    if s == 0:
-                        quant_ll(1)
-                    if ok(s - 1):
-                        exps(s - 1, 0)
-                    if ok(s + 1):
-                        q_copy(s + 1)
-                    if ok(s - 3):
-                        moments(s - 3)
-                    if ok(s - 1):
-                        exps(s - 1, 1)
-                    if s == 1:
-                        shift_copies(1)
-                    if ok(s - 1):
-                        exps(s - 1, 2)
-                    if ok(s - 2):
-                        one_over_den(s - 2)
-                divide(STEPS - 3)
-                exps(STEPS - 1, 0)
-                moments(STEPS - 3)
-                weigh(STEPS - 2, 0, 9)
-                one_over_den(STEPS - 2)
-                exps(STEPS - 1, 1)
-                exps(STEPS - 1, 2)
-                weigh(STEPS - 1, 0, 6)
-                divide(STEPS - 2)
-                moments(STEPS - 2)
-                weigh(STEPS - 1, 6, 9)
-                one_over_den(STEPS - 1)
-                nc.scalar.activation(out=warm[:], in_=rds[STEPS - 1][:, 0, 0:1], func=ACT.Sqrt)
-                divide(STEPS - 1)
-                moments(STEPS - 1)
-
-            tot = main.tile([P, 2, 4], F32, name="tot", tag="tot", bufs=1)
-            nc.vector.tensor_reduce(out=tot[:].rearrange("p k o -> p (k o)"),
-                                    in_=msums[:].rearrange("p k o s -> p (k o) s"),
-                                    axis=mybir.AxisListType.X, op=ALU.add)
-            avg = main.tile([P, 2, 4], F32, name="avg", tag="avg", bufs=1)
-            nc.vector.tensor_scalar(out=avg[:], in0=tot[:], scalar1=1.0 / NPIX, scalar2=None, op0=ALU.mult)
-            dd = main.tile([P, 4], F32, name="dd", tag="dd", bufs=1)
-            nc.vector.tensor_tensor(out=dd[:], in0=avg[:, 0, :], in1=avg[:, 0, :], op=ALU.mult)
-            var = main.tile([P, 4], F32, name="var", tag="var", bufs=1)
-            nc.vector.tensor_tensor(out=var[:], in0=avg[:, 1, :], in1=dd[:], op=ALU.subtract)
-            ve = main.tile([P, 4], F32, name="ve", tag="ve", bufs=1)
-            nc.vector.tensor_scalar(out=ve[:], in0=var[:], scalar1=BN_EPS, scalar2=None, op0=ALU.add)
-            mean = main.tile([P, 4], F32, name="mean", tag="mean", bufs=1)
-            nc.vector.tensor_tensor(out=mean[:], in0=avg[:, 0, :], in1=neg_pivot[:], op=ALU.subtract)
-            sd = main.tile([P, 4], F32, name="sd", tag="sd", bufs=1)
-            nc.scalar.activation(out=sd[:], in_=ve[:], func=ACT.Sqrt)
-            rstd = main.tile([P, 4], F32, name="rstd", tag="rstd", bufs=1)
-            nc.vector.reciprocal(out=rstd[:], in_=sd[:])
-            gain = main.tile([P, 4], F32, name="gain", tag="gain", bufs=1)
-            nc.vector.tensor_tensor(out=gain[:], in0=gam_bf[:], in1=rstd[:], op=ALU.mult)
-            mg = main.tile([P, 4], F32, name="mg", tag="mg", bufs=1)
-            nc.vector.tensor_tensor(out=mg[:], in0=mean[:], in1=gain[:], op=ALU.mult)
-            shift = main.tile([P, 4], F32, name="shift", tag="shift", bufs=1)
-            nc.vector.tensor_tensor(out=shift[:], in0=bet_bf[:], in1=mg[:], op=ALU.subtract)
-            out_v = out.rearrange("b (c r) h w -> c r b (h w)", r=4)
+        def moments(s, sums_on_vector=False):
+            cols = slice(P * s, P * (s + 1))
             for ob in range(4):
-                n = main.tile([P, NPIX], F32, name="n", tag="n")
-                nc.scalar.activation(out=n[:].rearrange("p (b y x) -> p b y x", b=NB, x=16),
-                                     in_=att[:, ob, :].rearrange("p (y b x) -> p b y x", b=NB, x=16),
-                                     func=ACT.Identity, bias=shift[:, ob:ob + 1], scale=gain[:, ob:ob + 1])
-                neg = main.tile([P, NPIX], F32, name="neg", tag="neg")
-                nc.vector.tensor_scalar(out=neg[:], in0=n[:], scalar1=0.0, scalar2=a_col[:, 0:1],
-                                        op0=ALU.min, op1=ALU.mult)
-                res = main.tile([P, NPIX], F32, name="res", tag="res")
-                nc.vector.scalar_tensor_tensor(out=res[:], in0=n[:], scalar=0.0, in1=neg[:],
-                                               op0=ALU.max, op1=ALU.add)
-                nc.sync.dma_start(out=out_v[:, ob], in_=res[:].rearrange("p (b f) -> p b f", b=NB))
+                if sums_on_vector:
+                    junk_v = main.tile([P, P], F32, name="junk_v", tag="junk_v")
+                    nc.vector.tensor_scalar(out=junk_v[:], in0=att[:, ob, cols], scalar1=neg_pivot[:, ob:ob + 1],
+                                            scalar2=None, op0=ALU.add, op1=ALU.add,
+                                            accum_out=msums[:, 0, ob, s:s + 1])
+                for kind, func in enumerate((ACT.Identity, ACT.Square)):
+                    if kind == 0 and sums_on_vector:
+                        continue
+                    junk = main.tile([P, P], F32, name="junk", tag="junk")
+                    nc.scalar.activation(out=junk[:], in_=att[:, ob, cols], func=func,
+                                         bias=neg_pivot[:, ob:ob + 1], scale=1.0,
+                                         accum_out=msums[:, kind, ob, s:s + 1])
+
+        g_c1 = weight_copies(W_C1)
+        quant_w(W_C1, g_c1)
+        nc.vector.memset(zeros_bf[:], 0.0)
+        for t in range(4):
+            nc.vector.tensor_scalar(out=bias_full[:, :, t], in0=zeros_bf[:], scalar1=bias_bf[:, t:t + 1],
+                                    scalar2=None, op0=ALU.add)
+        haar_from_pe(0)
+        quant_ll(0)
+        g_q = weight_copies(W_Q)
+        add_bias(0)
+        add_bias(1)
+        shift_copies(0, True)
+        g_k = weight_copies(W_K)
+        quant_y(0)
+        quant_w(W_Q, g_q)
+        quant_w(W_K, g_k)
+        q_copy(0)
+        haar_from_pe(1)
+
+        for s in range(STEPS):
+            scores(s)
+            if s == 0:
+                haar_on_vector(1, 2)
+                haar_on_vector(1, 3)
+            if s == 1:
+                quant_ll(2)
+            if ok(s - 3):
+                divide(s - 3)
+            if ok(s - 2):
+                weigh(s - 2, 0, 9)
+            if s == 2:
+                quant_y(2)
+            shift_by_max(s, LAST_ON_VECTOR if s == STEPS - 1 else 0)
+            if s == 0:
+                quant_ll(1)
+            if ok(s - 1):
+                exps(s - 1, 0)
+            if ok(s + 1):
+                q_copy(s + 1)
+            if s == 0:
+                add_bias(2)
+                add_bias(3)
+                shift_copies(1, True)
+                quant_y(1)
+                g_v = weight_copies(W_V)
+                haar_from_pe(2)
+                for b in range(NB):
+                    haar_on_vector(2, b)
+                quant_w(W_V, g_v)
+                nc.vector.tensor_copy(out=a_col[:], in_=a_bf[:])
+            if s == 1:
+                for r in range(4, 8):
+                    add_bias(r)
+            if ok(s - 3):
+                moments(s - 3)
+            if ok(s - 1):
+                exps(s - 1, 1)
+            if ok(s - 1):
+                exps(s - 1, 2)
+            if s == 1:
+                shift_copies(2, False)
+            if ok(s - 2):
+                one_over_den(s - 2)
+        divide(STEPS - 3)
+        exps(STEPS - 1, 0)
+        moments(STEPS - 3)
+        weigh(STEPS - 2, 0, 9)
+        exps(STEPS - 1, 1)
+        exps(STEPS - 1, 2)
+        weigh(STEPS - 1, 0, 9)
+        log_den(STEPS - 2)
+        log_den(STEPS - 1)
+        exp_minus_log(STEPS - 2)
+        exp_minus_log(STEPS - 1)
+        divide(STEPS - 2)
+        moments(STEPS - 2, True)
+        divide(STEPS - 1)
+        moments(STEPS - 1, True)
+        nc.scalar.activation(out=warm[:], in_=rds[STEPS - 1][:, 0, 0:1], func=ACT.Sqrt)
+
+        tot = main.tile([P, 2, 4], F32, name="tot", tag="tot", bufs=1)
+        nc.vector.tensor_reduce(out=tot[:].rearrange("p k o -> p (k o)"),
+                                in_=msums[:].rearrange("p k o s -> p (k o) s"),
+                                axis=mybir.AxisListType.X, op=ALU.add)
+        dd = main.tile([P, 4], F32, name="dd", tag="dd", bufs=1)
+        nc.vector.scalar_tensor_tensor(out=dd[:], in0=tot[:, 0, :], scalar=1.0 / (NPIX * NPIX), in1=tot[:, 0, :],
+                                       op0=ALU.mult, op1=ALU.mult)
+        var = main.tile([P, 4], F32, name="var", tag="var", bufs=1)
+        nc.vector.scalar_tensor_tensor(out=var[:], in0=tot[:, 1, :], scalar=1.0 / NPIX, in1=dd[:],
+                                       op0=ALU.mult, op1=ALU.subtract)
+        ve = main.tile([P, 4], F32, name="ve", tag="ve", bufs=1)
+        nc.vector.tensor_scalar(out=ve[:], in0=var[:], scalar1=BN_EPS, scalar2=None, op0=ALU.add)
+        sd = main.tile([P, 4], F32, name="sd", tag="sd", bufs=1)
+        nc.scalar.activation(out=sd[:], in_=ve[:], func=ACT.Sqrt)
+        neg_mean = main.tile([P, 4], F32, name="neg_mean", tag="neg_mean", bufs=1)
+        nc.vector.scalar_tensor_tensor(out=neg_mean[:], in0=tot[:, 0, :], scalar=-1.0 / NPIX, in1=neg_pivot[:],
+                                       op0=ALU.mult, op1=ALU.add)
+        nmg = main.tile([P, 4], F32, name="nmg", tag="nmg", bufs=1)
+        nc.vector.tensor_tensor(out=nmg[:], in0=neg_mean[:], in1=gam_bf[:], op=ALU.mult)
+        rstd = main.tile([P, 4], F32, name="rstd", tag="rstd", bufs=1)
+        nc.vector.reciprocal(out=rstd[:], in_=sd[:])
+        mg = main.tile([P, 4], F32, name="mg", tag="mg", bufs=1)
+        nc.vector.tensor_tensor(out=mg[:], in0=nmg[:], in1=rstd[:], op=ALU.mult)
+        gain = main.tile([P, 4], F32, name="gain", tag="gain", bufs=1)
+        nc.vector.tensor_tensor(out=gain[:], in0=gam_bf[:], in1=rstd[:], op=ALU.mult)
+        shift = main.tile([P, 4], F32, name="shift", tag="shift", bufs=1)
+        nc.vector.tensor_tensor(out=shift[:], in0=bet_bf[:], in1=mg[:], op=ALU.add)
+        out_v = out.rearrange("b (c r) h w -> c r b (h w)", r=4)
+        for ob in range(4):
+            n = main.tile([P, NPIX], F32, name="n", tag="z", bufs=3)
+            nc.scalar.activation(out=n[:].rearrange("p (b y x) -> p b y x", b=NB, x=16),
+                                 in_=att[:, ob, :].rearrange("p (y b x) -> p b y x", b=NB, x=16),
+                                 func=ACT.Identity, bias=shift[:, ob:ob + 1], scale=gain[:, ob:ob + 1])
+            neg = main.tile([P, NPIX], F32, name="neg", tag="ev", bufs=2)
+            nc.vector.tensor_scalar(out=neg[:], in0=n[:], scalar1=0.0, scalar2=a_col[:, 0:1],
+                                    op0=ALU.min, op1=ALU.mult)
+            res = mid.tile([P, NPIX], F32, name="res", tag=("ll", "y_mid", "y_left", "y_right")[ob], align_bytes=64)
+            nc.vector.scalar_tensor_tensor(out=res[:], in0=n[:], scalar=0.0, in1=neg[:],
+                                           op0=ALU.max, op1=ALU.add)
+            nc.sync.dma_start(out=out_v[:, ob], in_=res[:].rearrange("p (b f) -> p b f", b=NB))

@@ -274,15 +274,19 @@ def tile_merge_pa_kernel(tc, x, w_c1, b_c1, w_q, w_k, w_v, bn_gamma, bn_beta, pr
                 pump_to(tok)
                 halve(pc, tok[2], banks[tok][:, 0:ROW * PIECES[pc][1]])
 
-        def haar_on_vector(pc, b):
+        def haar_on_vector(pc, images):
             nr = PIECES[pc][1]
-            rows = x_piece(pc, b).rearrange("p j (i a w) -> p j i a w", a=2, w=32)
-            s1 = main.tile([P, 4, nr, 32], F32, name="s1", tag="s1", bufs=2)
-            nc.vector.tensor_tensor(out=s1[:], in0=rows[:, :, :, 0, :], in1=rows[:, :, :, 1, :], op=ALU.add)
-            pairs = s1[:].rearrange("p j i (x e) -> p (j i x) e", e=2)
-            s2 = main.tile([P, ROW * nr], F32, name="s2", tag="s2", bufs=2)
-            nc.vector.tensor_tensor(out=s2[:], in0=pairs[:, :, 0], in1=pairs[:, :, 1], op=ALU.add)
-            halve(pc, b, s2[:])
+            row_sums = []
+            for b in images:
+                rows = x_piece(pc, b).rearrange("p j (i a w) -> p j i a w", a=2, w=32)
+                s1 = main.tile([P, 4, nr, 32], F32, name="s1", tag="s1", bufs=2)
+                nc.vector.tensor_tensor(out=s1[:], in0=rows[:, :, :, 0, :], in1=rows[:, :, :, 1, :], op=ALU.add)
+                row_sums.append(s1)
+            for b, s1 in zip(images, row_sums):
+                pairs = s1[:].rearrange("p j i (x e) -> p (j i x) e", e=2)
+                s2 = main.tile([P, ROW * nr], F32, name="s2", tag="s2", bufs=2)
+                nc.vector.tensor_tensor(out=s2[:], in0=pairs[:, :, 0], in1=pairs[:, :, 1], op=ALU.add)
+                halve(pc, b, s2[:])
 
         def quant_ll(pc):
             c0 = ROW * PIECES[pc][0]
@@ -319,21 +323,25 @@ def tile_merge_pa_kernel(tc, x, w_c1, b_c1, w_q, w_k, w_v, bn_gamma, bn_beta, pr
             nc.scalar.copy(out=q_sb[:], in_=banks[("q", s, 0)][:])
             q_sbs[s] = q_sb
 
-        def scores(s):
-            z = main.tile([P, 9, 512], F32, name="z", tag="z", bufs=3)
-            zs[s] = z
-            for j in range(9):
+        def scores(s, j0, j1):
+            if j0 == 0:
+                z = main.tile([P, 9, 512], F32, name="z", tag="z", bufs=3)
+                zs[s] = z
+            for j in range(j0, j1):
                 pump_to(("k", s, j))
-                nc.vector.tensor_tensor(out=z[:, j, :], in0=q_sbs[s][:], in1=banks[("k", s, j)][:], op=ALU.mult)
+                nc.vector.tensor_tensor(out=zs[s][:, j, :], in0=q_sbs[s][:], in1=banks[("k", s, j)][:], op=ALU.mult)
 
-        def shift_by_max(s, on_vector=0):
+        def shift_by_max(s, between, on_vector=0):
             z = zs[s]
             t1 = main.tile([P, 4, 512], F32, name="t1", tag="t1", bufs=1)
             nc.vector.tensor_tensor(out=t1[:], in0=z[:, 0:4, :], in1=z[:, 4:8, :], op=ALU.max)
+            between[0]()
             t2 = main.tile([P, 2, 512], F32, name="t2", tag="t2", bufs=1)
             nc.vector.tensor_tensor(out=t2[:], in0=t1[:, 0:2, :], in1=t1[:, 2:4, :], op=ALU.max)
+            between[1]()
             t3 = main.tile([P, 512], F32, name="t3", tag="t3", bufs=1)
             nc.vector.tensor_tensor(out=t3[:], in0=t2[:, 0, :], in1=t2[:, 1, :], op=ALU.max)
+            between[2]()
             m = main.tile([P, 512], F32, name="m", tag="m")
             nc.vector.tensor_tensor(out=m[:], in0=t3[:], in1=z[:, 8, :], op=ALU.max)
             for j in range(on_vector):
@@ -393,9 +401,9 @@ def tile_merge_pa_kernel(tc, x, w_c1, b_c1, w_q, w_k, w_v, bn_gamma, bn_beta, pr
                                          bias=neg_pivot[:, ob:ob + 1], scale=1.0,
                                          accum_out=msums[:, kind, ob, s:s + 1])
 
+        nc.vector.memset(zeros_bf[:], 0.0)
         g_c1 = weight_copies(W_C1)
         quant_w(W_C1, g_c1)
-        nc.vector.memset(zeros_bf[:], 0.0)
         for t in range(4):
             nc.vector.tensor_scalar(out=bias_full[:, :, t], in0=zeros_bf[:], scalar1=bias_bf[:, t:t + 1],
                                     scalar2=None, op0=ALU.add)
@@ -404,34 +412,46 @@ def tile_merge_pa_kernel(tc, x, w_c1, b_c1, w_q, w_k, w_v, bn_gamma, bn_beta, pr
         g_q = weight_copies(W_Q)
         add_bias(0)
         add_bias(1)
+        quant_w(W_Q, g_q)
         shift_copies(0, True)
         g_k = weight_copies(W_K)
         quant_y(0)
-        quant_w(W_Q, g_q)
         quant_w(W_K, g_k)
         q_copy(0)
         haar_from_pe(1)
 
+        def nothing():
+            return None
+
+        def early_scores(s, j):
+            return (lambda: scores(s, j, j + 1)) if ok(s) else nothing
+
+        scores(0, 0, AHEAD)
         for s in range(STEPS):
-            scores(s)
+            scores(s, AHEAD, 9)
             if s == 0:
-                haar_on_vector(1, 2)
-                haar_on_vector(1, 3)
+                haar_on_vector(1, (2, 3))
             if s == 1:
                 quant_ll(2)
+            if ok(s - 1):
+                exps(s - 1, 0)
+            if s > 0 and ok(s + 1):
+                q_copy(s + 1)
             if ok(s - 3):
                 divide(s - 3)
             if ok(s - 2):
                 weigh(s - 2, 0, 9)
             if s == 2:
                 quant_y(2)
-            shift_by_max(s, LAST_ON_VECTOR if s == STEPS - 1 else 0)
             if s == 0:
-                quant_ll(1)
-            if ok(s - 1):
-                exps(s - 1, 0)
-            if ok(s + 1):
+                shift_by_max(s, (lambda: quant_ll(1), nothing, nothing))
                 q_copy(s + 1)
+            elif s == 1:
+                shift_by_max(s, (lambda: (add_bias(4), add_bias(5)), lambda: add_bias(6), lambda: add_bias(7)))
+                scores(s + 1, 0, AHEAD)
+            else:
+                shift_by_max(s, (early_scores(s + 1, 0), early_scores(s + 1, 1), early_scores(s + 1, 2)),
+                             LAST_ON_VECTOR if s == STEPS - 1 else 0)
             if s == 0:
                 add_bias(2)
                 add_bias(3)
@@ -439,13 +459,11 @@ def tile_merge_pa_kernel(tc, x, w_c1, b_c1, w_q, w_k, w_v, bn_gamma, bn_beta, pr
                 quant_y(1)
                 g_v = weight_copies(W_V)
                 haar_from_pe(2)
-                for b in range(NB):
-                    haar_on_vector(2, b)
+                haar_on_vector(2, (0, 1))
+                haar_on_vector(2, (2, 3))
                 quant_w(W_V, g_v)
                 nc.vector.tensor_copy(out=a_col[:], in_=a_bf[:])
-            if s == 1:
-                for r in range(4, 8):
-                    add_bias(r)
+                scores(1, 0, AHEAD)
             if ok(s - 3):
                 moments(s - 3)
             if ok(s - 1):
@@ -501,15 +519,34 @@ def tile_merge_pa_kernel(tc, x, w_c1, b_c1, w_q, w_k, w_v, bn_gamma, bn_beta, pr
         shift = main.tile([P, 4], F32, name="shift", tag="shift", bufs=1)
         nc.vector.tensor_tensor(out=shift[:], in0=bet_bf[:], in1=mg[:], op=ALU.add)
         out_v = out.rearrange("b (c r) h w -> c r b (h w)", r=4)
-        for ob in range(4):
+        ns = {}
+        negs = {}
+
+        def normalise(ob):
             n = main.tile([P, NPIX], F32, name="n", tag="z", bufs=3)
             nc.scalar.activation(out=n[:].rearrange("p (b y x) -> p b y x", b=NB, x=16),
                                  in_=att[:, ob, :].rearrange("p (y b x) -> p b y x", b=NB, x=16),
                                  func=ACT.Identity, bias=shift[:, ob:ob + 1], scale=gain[:, ob:ob + 1])
+            ns[ob] = n
+
+        def negative_part(ob):
             neg = main.tile([P, NPIX], F32, name="neg", tag="ev", bufs=2)
-            nc.vector.tensor_scalar(out=neg[:], in0=n[:], scalar1=0.0, scalar2=a_col[:, 0:1],
+            nc.vector.tensor_scalar(out=neg[:], in0=ns[ob][:], scalar1=0.0, scalar2=a_col[:, 0:1],
                                     op0=ALU.min, op1=ALU.mult)
+            negs[ob] = neg
+
+        def prelu_and_store(ob):
             res = mid.tile([P, NPIX], F32, name="res", tag=("ll", "y_mid", "y_left", "y_right")[ob], align_bytes=64)
-            nc.vector.scalar_tensor_tensor(out=res[:], in0=n[:], scalar=0.0, in1=neg[:],
+            nc.vector.scalar_tensor_tensor(out=res[:], in0=ns[ob][:], scalar=0.0, in1=negs[ob][:],
                                            op0=ALU.max, op1=ALU.add)
             nc.sync.dma_start(out=out_v[:, ob], in_=res[:].rearrange("p (b f) -> p b f", b=NB))
+
+        normalise(0)
+        normalise(1)
+        negative_part(0)
+        for ob in range(4):
+            if ob + 2 < 4:
+                normalise(ob + 2)
+            if ob + 1 < 4:
+                negative_part(ob + 1)
+            prelu_and_store(ob)

@@ -344,10 +344,10 @@ def tile_merge_pa_kernel(tc, x, w_c1, b_c1, w_q, w_k, w_v, bn_gamma, bn_beta, pr
             between[2]()
             m = main.tile([P, 512], F32, name="m", tag="m")
             nc.vector.tensor_tensor(out=m[:], in0=t3[:], in1=z[:, 8, :], op=ALU.max)
-            for j in range(on_vector):
-                nc.vector.tensor_tensor(out=z[:, j, :], in0=z[:, j, :], in1=m[:], op=ALU.subtract)
-            for j in range(on_vector, 9):
-                nc.gpsimd.tensor_tensor(out=z[:, j, :], in0=z[:, j, :], in1=m[:], op=ALU.subtract)
+            m_thrice = m[:].unsqueeze(1).to_broadcast([P, 3, 512])
+            for g in range(3):
+                eng = nc.vector if 3 * g < on_vector else nc.gpsimd
+                eng.tensor_tensor(out=z[:, 3 * g:3 * g + 3, :], in0=z[:, 3 * g:3 * g + 3, :], in1=m_thrice, op=ALU.subtract)
 
         def exps(s, g):
             z = zs[s]

@@ -22,7 +22,7 @@ AHEAD = 3
 T_BURST = 6
 LAST_ON_VECTOR = 3
 PIECES = ((0, 4), (4, 4), (8, 8))
-HAAR_ON_VECTOR = ((1, 2), (1, 3), (2, 0), (2, 1), (2, 2), (2, 3))
+HAAR_ON_VECTOR = ((0, 0), (0, 1), (1, 2), (1, 3), (2, 0), (2, 1), (2, 2))
 W_C1, W_K, W_Q, W_V = 0, 1, 2, 3
 
 FLOPS = 4 * 2 * 512 * 512 * 1024
@@ -97,7 +97,10 @@ def tile_merge_pa_kernel(tc, x, w_c1, b_c1, w_q, w_k, w_v, bn_gamma, bn_beta, pr
             y_scales.append(yst)
 
         att = keep.tile([P, 4, NPIX], F32, name="att")
-        msums = keep.tile([P, 2, 4, STEPS], F32, name="msums")
+        msums = keep.tile([P, 2, 4, STEPS + 1], F32, name="msums")
+        nc.vector.memset(msums[:, :, :, STEPS], 0.0)
+        nc.vector.tensor_scalar(out=msums[:, 1, :, STEPS], in0=msums[:, 1, :, STEPS], scalar1=NPIX * BN_EPS, scalar2=None,
+                                op0=ALU.add)
         neg_pivot = keep.tile([P, 4], F32, name="neg_pivot")
         a_col = keep.tile([P, 1], F32, name="a_col")
         zeros_bf = keep.tile([P, P], BF16, name="zeros_bf")
@@ -171,6 +174,18 @@ def tile_merge_pa_kernel(tc, x, w_c1, b_c1, w_q, w_k, w_v, bn_gamma, bn_beta, pr
                 bank = psm.tile([P, 4, P], BANK_DT, name="bank", tag="v_ps", bufs=3)
                 first_conv(bank, s)
                 banks[tok] = bank
+            elif kind == "C":
+                c0 = ROW * PIECES[s][0]
+                n = ROW * PIECES[s][1]
+                if j == 3:
+                    wide = psm.tile([P, n], BANK_DT, name="wide_last", tag="den", bufs=1)
+                else:
+                    wide = psm.tile([P, n], BANK_DT, name="wide", tag="v_ps", bufs=3)
+                nc.tensor.matmul_mx(out=wide[:], lhsT=w_codes[W_C1][:, P * j:P * (j + 1)].bitcast(FP8X4),
+                                    lhsT_scale=w_scales[W_C1][:, P * j:P * (j + 1)],
+                                    rhs=ll_codes[:, c0:c0 + n].bitcast(FP8X4), rhs_scale=ll_scales[:, c0:c0 + n],
+                                    start=True, stop=True)
+                banks[tok] = wide
             elif kind == "w":
                 words = w_all[:, s].bitcast(F32)
                 wT = psm.tile([P, 2, 2, P], F32, name="wT", tag=("k_ps" if s != W_V else "v_ps"), bufs=3)
@@ -219,9 +234,9 @@ def tile_merge_pa_kernel(tc, x, w_c1, b_c1, w_q, w_k, w_v, bn_gamma, bn_beta, pr
             if ok(s + 1):
                 mms.append(("q", s + 1, 0))
             if s == 0:
-                mms.extend([("c", 2, 0), ("c", 3, 0), ("w", W_V, 0), ("w", W_V, 1)] + on_pe(2))
+                mms.extend([("C", 1, t) for t in range(4)] + [("w", W_V, 0), ("w", W_V, 1)] + on_pe(2))
             if s == 1:
-                mms.extend([("c", r, 0) for r in range(4, 8)])
+                mms.extend([("C", 2, t) for t in range(4)])
             sums = []
             if ok(s - 2):
                 mms.extend([("v", s - 2, j) for j in range(AHEAD, 9)])
@@ -298,6 +313,14 @@ def tile_merge_pa_kernel(tc, x, w_c1, b_c1, w_q, w_k, w_v, bn_gamma, bn_beta, pr
             pump_to(("c", r, 0))
             nc.vector.tensor_tensor(out=y_mid[:, P * r:P * (r + 1), :], in0=banks[("c", r, 0)][:].rearrange("p t n -> p n t"),
                                     in1=bias_full[:], op=ALU.add)
+
+        def add_bias_on_scalar(pc):
+            c0 = ROW * PIECES[pc][0]
+            n = ROW * PIECES[pc][1]
+            for t in range(4):
+                pump_to(("C", pc, t))
+                nc.scalar.activation(out=y_mid[:, c0:c0 + n, t], in_=banks[("C", pc, t)][:], func=ACT.Identity,
+                                     bias=bias_bf[:, t:t + 1], scale=1.0)
 
         def shift_copies(pc, on_vector):
             g0 = NB * PIECES[pc][0]
@@ -403,6 +426,7 @@ def tile_merge_pa_kernel(tc, x, w_c1, b_c1, w_q, w_k, w_v, bn_gamma, bn_beta, pr
 
         nc.vector.memset(zeros_bf[:], 0.0)
         g_c1 = weight_copies(W_C1)
+        haar_on_vector(0, (0, 1))
         quant_w(W_C1, g_c1)
         for t in range(4):
             nc.vector.tensor_scalar(out=bias_full[:, :, t], in0=zeros_bf[:], scalar1=bias_bf[:, t:t + 1],
@@ -431,8 +455,6 @@ def tile_merge_pa_kernel(tc, x, w_c1, b_c1, w_q, w_k, w_v, bn_gamma, bn_beta, pr
             scores(s, AHEAD, 9)
             if s == 0:
                 haar_on_vector(1, (2, 3))
-            if s == 1:
-                quant_ll(2)
             if ok(s - 1):
                 exps(s - 1, 0)
             if s > 0 and ok(s + 1):
@@ -444,25 +466,20 @@ def tile_merge_pa_kernel(tc, x, w_c1, b_c1, w_q, w_k, w_v, bn_gamma, bn_beta, pr
             if s == 2:
                 quant_y(2)
             if s == 0:
-                shift_by_max(s, (lambda: quant_ll(1), nothing, nothing))
-                q_copy(s + 1)
+                shift_by_max(s, (lambda: (quant_ll(1), q_copy(1), add_bias_on_scalar(1), shift_copies(1, False)),
+                                 lambda: haar_on_vector(2, (0, 1)), lambda: haar_on_vector(2, (2,))))
             elif s == 1:
-                shift_by_max(s, (lambda: (add_bias(4), add_bias(5)), lambda: add_bias(6), lambda: add_bias(7)))
+                shift_by_max(s, (lambda: quant_ll(2), lambda: quant_w(W_V, g_v),
+                                 lambda: nc.vector.tensor_copy(out=a_col[:], in_=a_bf[:])))
+                add_bias_on_scalar(2)
                 scores(s + 1, 0, AHEAD)
             else:
                 shift_by_max(s, (early_scores(s + 1, 0), early_scores(s + 1, 1), early_scores(s + 1, 2)),
                              LAST_ON_VECTOR if s == STEPS - 1 else 0)
             if s == 0:
-                add_bias(2)
-                add_bias(3)
-                shift_copies(1, True)
-                quant_y(1)
                 g_v = weight_copies(W_V)
                 haar_from_pe(2)
-                haar_on_vector(2, (0, 1))
-                haar_on_vector(2, (2, 3))
-                quant_w(W_V, g_v)
-                nc.vector.tensor_copy(out=a_col[:], in_=a_bf[:])
+                quant_y(1)
                 scores(1, 0, AHEAD)
             if ok(s - 3):
                 moments(s - 3)
@@ -498,11 +515,9 @@ def tile_merge_pa_kernel(tc, x, w_c1, b_c1, w_q, w_k, w_v, bn_gamma, bn_beta, pr
         dd = main.tile([P, 4], F32, name="dd", tag="dd", bufs=1)
         nc.vector.scalar_tensor_tensor(out=dd[:], in0=tot[:, 0, :], scalar=1.0 / (NPIX * NPIX), in1=tot[:, 0, :],
                                        op0=ALU.mult, op1=ALU.mult)
-        var = main.tile([P, 4], F32, name="var", tag="var", bufs=1)
-        nc.vector.scalar_tensor_tensor(out=var[:], in0=tot[:, 1, :], scalar=1.0 / NPIX, in1=dd[:],
-                                       op0=ALU.mult, op1=ALU.subtract)
         ve = main.tile([P, 4], F32, name="ve", tag="ve", bufs=1)
-        nc.vector.tensor_scalar(out=ve[:], in0=var[:], scalar1=BN_EPS, scalar2=None, op0=ALU.add)
+        nc.vector.scalar_tensor_tensor(out=ve[:], in0=tot[:, 1, :], scalar=1.0 / NPIX, in1=dd[:],
+                                       op0=ALU.mult, op1=ALU.subtract)
         sd = main.tile([P, 4], F32, name="sd", tag="sd", bufs=1)
         nc.scalar.activation(out=sd[:], in_=ve[:], func=ACT.Sqrt)
         neg_mean = main.tile([P, 4], F32, name="neg_mean", tag="neg_mean", bufs=1)

@@ -178,7 +178,7 @@ def tile_merge_pa_kernel(tc, x, w_c1, b_c1, w_q, w_k, w_v, bn_gamma, bn_beta, pr
                 c0 = ROW * PIECES[s][0]
                 n = ROW * PIECES[s][1]
                 if j == 3:
-                    wide = psm.tile([P, n], BANK_DT, name="wide_last", tag="den", bufs=1)
+                    wide = psm.tile([P, n], BANK_DT, name="wide_last", tag="num", bufs=1)
                 else:
                     wide = psm.tile([P, n], BANK_DT, name="wide", tag="v_ps", bufs=3)
                 nc.tensor.matmul_mx(out=wide[:], lhsT=w_codes[W_C1][:, P * j:P * (j + 1)].bitcast(FP8X4),
@@ -239,7 +239,7 @@ def tile_merge_pa_kernel(tc, x, w_c1, b_c1, w_q, w_k, w_v, bn_gamma, bn_beta, pr
                 mms.extend([("C", 2, t) for t in range(4)])
             sums = []
             if ok(s - 2):
-                mms.extend([("v", s - 2, j) for j in range(AHEAD, 9)])
+                mms.extend([("v", s - 2, j) for j in range(0 if s == 2 else AHEAD, 9)])
                 sums = [("F", s - 2, i) for i in range(36)]
             if s == STEPS:
                 pe_list.extend(sums)
@@ -252,7 +252,7 @@ def tile_merge_pa_kernel(tc, x, w_c1, b_c1, w_q, w_k, w_v, bn_gamma, bn_beta, pr
             pe_list.extend(sums)
             if ok(s + 1):
                 pe_list.extend([("k", s + 1, j) for j in range(AHEAD)])
-            if ok(s - 1):
+            if ok(s - 1) and s != 1:
                 pe_list.extend([("v", s - 1, j) for j in range(AHEAD)])
             if ok(s - 2):
                 pe_list.extend([("G", s - 2, i) for i in range(36)])
@@ -299,7 +299,7 @@ def tile_merge_pa_kernel(tc, x, w_c1, b_c1, w_q, w_k, w_v, bn_gamma, bn_beta, pr
                 row_sums.append(s1)
             for b, s1 in zip(images, row_sums):
                 pairs = s1[:].rearrange("p j i (x e) -> p (j i x) e", e=2)
-                s2 = main.tile([P, ROW * nr], F32, name="s2", tag="s2", bufs=2)
+                s2 = main.tile([P, ROW * nr], F32, name="s2", tag="s2", bufs=3)
                 nc.vector.tensor_tensor(out=s2[:], in0=pairs[:, :, 0], in1=pairs[:, :, 1], op=ALU.add)
                 halve(pc, b, s2[:])
 
@@ -471,7 +471,6 @@ def tile_merge_pa_kernel(tc, x, w_c1, b_c1, w_q, w_k, w_v, bn_gamma, bn_beta, pr
             elif s == 1:
                 shift_by_max(s, (lambda: quant_ll(2), lambda: quant_w(W_V, g_v),
                                  lambda: nc.vector.tensor_copy(out=a_col[:], in_=a_bf[:])))
-                add_bias_on_scalar(2)
                 scores(s + 1, 0, AHEAD)
             else:
                 shift_by_max(s, (early_scores(s + 1, 0), early_scores(s + 1, 1), early_scores(s + 1, 2)),
@@ -488,6 +487,7 @@ def tile_merge_pa_kernel(tc, x, w_c1, b_c1, w_q, w_k, w_v, bn_gamma, bn_beta, pr
             if ok(s - 1):
                 exps(s - 1, 2)
             if s == 1:
+                add_bias_on_scalar(2)
                 shift_copies(2, False)
             if ok(s - 2):
                 one_over_den(s - 2)
@@ -503,8 +503,8 @@ def tile_merge_pa_kernel(tc, x, w_c1, b_c1, w_q, w_k, w_v, bn_gamma, bn_beta, pr
         exp_minus_log(STEPS - 2)
         exp_minus_log(STEPS - 1)
         divide(STEPS - 2)
-        moments(STEPS - 2, True)
         divide(STEPS - 1)
+        moments(STEPS - 2, True)
         moments(STEPS - 1, True)
         nc.scalar.activation(out=warm[:], in_=rds[STEPS - 1][:, 0, 0:1], func=ACT.Sqrt)
 
@@ -527,12 +527,12 @@ def tile_merge_pa_kernel(tc, x, w_c1, b_c1, w_q, w_k, w_v, bn_gamma, bn_beta, pr
         nc.vector.tensor_tensor(out=nmg[:], in0=neg_mean[:], in1=gam_bf[:], op=ALU.mult)
         rstd = main.tile([P, 4], F32, name="rstd", tag="rstd", bufs=1)
         nc.vector.reciprocal(out=rstd[:], in_=sd[:])
-        mg = main.tile([P, 4], F32, name="mg", tag="mg", bufs=1)
-        nc.vector.tensor_tensor(out=mg[:], in0=nmg[:], in1=rstd[:], op=ALU.mult)
         gain = main.tile([P, 4], F32, name="gain", tag="gain", bufs=1)
         nc.vector.tensor_tensor(out=gain[:], in0=gam_bf[:], in1=rstd[:], op=ALU.mult)
         shift = main.tile([P, 4], F32, name="shift", tag="shift", bufs=1)
-        nc.vector.tensor_tensor(out=shift[:], in0=bet_bf[:], in1=mg[:], op=ALU.add)
+        for ob in range(4):
+            nc.vector.scalar_tensor_tensor(out=shift[:, ob:ob + 1], in0=nmg[:, ob:ob + 1], scalar=rstd[:, ob:ob + 1],
+                                           in1=bet_bf[:, ob:ob + 1], op0=ALU.mult, op1=ALU.add)
         out_v = out.rearrange("b (c r) h w -> c r b (h w)", r=4)
         ns = {}
         negs = {}

@@ -97,10 +97,10 @@ def tile_merge_pa_kernel(tc, x, w_c1, b_c1, w_q, w_k, w_v, bn_gamma, bn_beta, pr
             y_scales.append(yst)
 
         att = keep.tile([P, 4, NPIX], F32, name="att")
-        msums = keep.tile([P, 2, 4, STEPS + 1], F32, name="msums")
-        nc.vector.memset(msums[:, :, :, STEPS], 0.0)
-        nc.vector.tensor_scalar(out=msums[:, 1, :, STEPS], in0=msums[:, 1, :, STEPS], scalar1=NPIX * BN_EPS, scalar2=None,
-                                op0=ALU.add)
+        msums = keep.tile([P, 2, 4, STEPS], F32, name="msums")
+        nc.vector.memset(msums[:, :, :, STEPS - 1], 0.0)
+        nc.vector.tensor_scalar(out=msums[:, 1, :, STEPS - 1], in0=msums[:, 1, :, STEPS - 1], scalar1=NPIX * BN_EPS,
+                                scalar2=None, op0=ALU.add)
         neg_pivot = keep.tile([P, 4], F32, name="neg_pivot")
         a_col = keep.tile([P, 1], F32, name="a_col")
         zeros_bf = keep.tile([P, P], BF16, name="zeros_bf")
@@ -254,8 +254,11 @@ def tile_merge_pa_kernel(tc, x, w_c1, b_c1, w_q, w_k, w_v, bn_gamma, bn_beta, pr
                 pe_list.extend([("k", s + 1, j) for j in range(AHEAD)])
             if ok(s - 1) and s != 1:
                 pe_list.extend([("v", s - 1, j) for j in range(AHEAD)])
-            if ok(s - 2):
+            if ok(s - 2) and s - 2 < STEPS - 2:
                 pe_list.extend([("G", s - 2, i) for i in range(36)])
+        for ob in range(4):
+            for s in (STEPS - 2, STEPS - 1):
+                pe_list.extend([("G", s, 9 * ob + j) for j in range(9)])
 
         done = set()
         pos = [0]
@@ -347,11 +350,11 @@ def tile_merge_pa_kernel(tc, x, w_c1, b_c1, w_q, w_k, w_v, bn_gamma, bn_beta, pr
             q_sbs[s] = q_sb
 
         def scores(s, j0, j1):
-            if j0 == 0:
-                z = main.tile([P, 9, 512], F32, name="z", tag="z", bufs=3)
-                zs[s] = z
             for j in range(j0, j1):
                 pump_to(("k", s, j))
+                if j == 0:
+                    z = main.tile([P, 9, 512], F32, name="z", tag="z", bufs=3)
+                    zs[s] = z
                 nc.vector.tensor_tensor(out=zs[s][:, j, :], in0=q_sbs[s][:], in1=banks[("k", s, j)][:], op=ALU.mult)
 
         def shift_by_max(s, between, on_vector=0):
@@ -388,12 +391,12 @@ def tile_merge_pa_kernel(tc, x, w_c1, b_c1, w_q, w_k, w_v, bn_gamma, bn_beta, pr
         def log_den(s):
             pump_to(("F", s, 35))
             lg = main.tile([P, 4, P], F32, name="lg", tag="lg")
-            nc.scalar.activation(out=lg[:], in_=dens[s][:], func=ACT.Ln)
+            nc.scalar.activation(out=lg[:], in_=dens[s][:], func=ACT.Abs_reciprocal_sqrt)
             lgs[s] = lg
 
         def exp_minus_log(s):
             rd = main.tile([P, 4, P], F32, name="rd", tag="rd")
-            nc.scalar.activation(out=rd[:], in_=lgs[s][:], func=ACT.Exp, scale=-1.0)
+            nc.scalar.activation(out=rd[:], in_=lgs[s][:], func=ACT.Square)
             rds[s] = rd
 
         def one_over_den(s):
@@ -502,50 +505,81 @@ def tile_merge_pa_kernel(tc, x, w_c1, b_c1, w_q, w_k, w_v, bn_gamma, bn_beta, pr
         log_den(STEPS - 1)
         exp_minus_log(STEPS - 2)
         exp_minus_log(STEPS - 1)
-        divide(STEPS - 2)
-        divide(STEPS - 1)
-        moments(STEPS - 2, True)
-        moments(STEPS - 1, True)
-        nc.scalar.activation(out=warm[:], in_=rds[STEPS - 1][:, 0, 0:1], func=ACT.Sqrt)
 
-        tot = main.tile([P, 2, 4], F32, name="tot", tag="tot", bufs=1)
-        nc.vector.tensor_reduce(out=tot[:].rearrange("p k o -> p (k o)"),
-                                in_=msums[:].rearrange("p k o s -> p (k o) s"),
-                                axis=mybir.AxisListType.X, op=ALU.add)
-        dd = main.tile([P, 4], F32, name="dd", tag="dd", bufs=1)
-        nc.vector.scalar_tensor_tensor(out=dd[:], in0=tot[:, 0, :], scalar=1.0 / (NPIX * NPIX), in1=tot[:, 0, :],
-                                       op0=ALU.mult, op1=ALU.mult)
-        ve = main.tile([P, 4], F32, name="ve", tag="ve", bufs=1)
-        nc.vector.scalar_tensor_tensor(out=ve[:], in0=tot[:, 1, :], scalar=1.0 / NPIX, in1=dd[:],
-                                       op0=ALU.mult, op1=ALU.subtract)
-        sd = main.tile([P, 4], F32, name="sd", tag="sd", bufs=1)
-        nc.scalar.activation(out=sd[:], in_=ve[:], func=ACT.Sqrt)
-        neg_mean = main.tile([P, 4], F32, name="neg_mean", tag="neg_mean", bufs=1)
-        nc.vector.scalar_tensor_tensor(out=neg_mean[:], in0=tot[:, 0, :], scalar=-1.0 / NPIX, in1=neg_pivot[:],
-                                       op0=ALU.mult, op1=ALU.add)
-        nmg = main.tile([P, 4], F32, name="nmg", tag="nmg", bufs=1)
-        nc.vector.tensor_tensor(out=nmg[:], in0=neg_mean[:], in1=gam_bf[:], op=ALU.mult)
-        rstd = main.tile([P, 4], F32, name="rstd", tag="rstd", bufs=1)
-        nc.vector.reciprocal(out=rstd[:], in_=sd[:])
-        gain = main.tile([P, 4], F32, name="gain", tag="gain", bufs=1)
-        nc.vector.tensor_tensor(out=gain[:], in0=gam_bf[:], in1=rstd[:], op=ALU.mult)
-        shift = main.tile([P, 4], F32, name="shift", tag="shift", bufs=1)
-        for ob in range(4):
-            nc.vector.scalar_tensor_tensor(out=shift[:, ob:ob + 1], in0=nmg[:, ob:ob + 1], scalar=rstd[:, ob:ob + 1],
-                                           in1=bet_bf[:, ob:ob + 1], op0=ALU.mult, op1=ALU.add)
+        last = slice(P * (STEPS - 2), NPIX)
+        tot = keep.tile([P, 2, 4], F32, name="tot")
+        dd = keep.tile([P, 4], F32, name="dd")
+        ve = keep.tile([P, 4], F32, name="ve")
+        neg_mean = keep.tile([P, 4], F32, name="neg_mean")
+        nmg = keep.tile([P, 4], F32, name="nmg")
+        rstd = keep.tile([P, 4], F32, name="rstd")
+        gain = keep.tile([P, 4], F32, name="gain")
+        shift = keep.tile([P, 4], F32, name="shift")
         out_v = out.rearrange("b (c r) h w -> c r b (h w)", r=4)
         ns = {}
         negs = {}
 
+        def col(t, ob):
+            return t[:, ob:ob + 1]
+
+        def divide_block(s, ob):
+            pump_to(("G", s, 9 * ob + 8))
+            nc.vector.tensor_tensor(out=att[:, ob, P * s:P * (s + 1)], in0=nums[s][:, ob, :], in1=rds[s][:, ob, :], op=ALU.mult)
+
+        def last_sum(ob):
+            junk_v = main.tile([P, 2 * P], F32, name="junk_v", tag="junk_v")
+            nc.vector.tensor_scalar(out=junk_v[:], in0=att[:, ob, last], scalar1=col(neg_pivot, ob), scalar2=None,
+                                    op0=ALU.add, op1=ALU.add, accum_out=msums[:, 0, ob, STEPS - 2:STEPS - 1])
+
+        def last_squares(ob):
+            junk = main.tile([P, 2 * P], F32, name="junk2", tag="junk2")
+            nc.scalar.activation(out=junk[:], in_=att[:, ob, last], func=ACT.Square, bias=col(neg_pivot, ob), scale=1.0,
+                                 accum_out=msums[:, 1, ob, STEPS - 2:STEPS - 1])
+
+        def pair(t, g):
+            return t[:, 2 * g:2 * g + 2]
+
+        def totals(g):
+            nc.vector.tensor_reduce(out=tot[:, :, 2 * g:2 * g + 2], in_=msums[:, :, 2 * g:2 * g + 2, :],
+                                    axis=mybir.AxisListType.X, op=ALU.add)
+
+        def mean_squared(g):
+            nc.vector.scalar_tensor_tensor(out=pair(dd, g), in0=tot[:, 0, 2 * g:2 * g + 2], scalar=1.0 / (NPIX * NPIX),
+                                           in1=tot[:, 0, 2 * g:2 * g + 2], op0=ALU.mult, op1=ALU.mult)
+
+        def var_plus_eps(g):
+            nc.vector.scalar_tensor_tensor(out=pair(ve, g), in0=tot[:, 1, 2 * g:2 * g + 2], scalar=1.0 / NPIX, in1=pair(dd, g),
+                                           op0=ALU.mult, op1=ALU.subtract)
+
+        def std(g):
+            nc.scalar.activation(out=pair(rstd, g), in_=pair(ve, g), func=ACT.Abs_reciprocal_sqrt)
+
+        def minus_mean(g):
+            nc.vector.scalar_tensor_tensor(out=pair(neg_mean, g), in0=tot[:, 0, 2 * g:2 * g + 2], scalar=-1.0 / NPIX,
+                                           in1=pair(neg_pivot, g), op0=ALU.mult, op1=ALU.add)
+
+        def minus_mean_gamma(g):
+            nc.vector.tensor_tensor(out=pair(nmg, g), in0=pair(neg_mean, g), in1=pair(gam_bf, g), op=ALU.mult)
+
+        def gain_of(g):
+            nc.vector.tensor_tensor(out=pair(gain, g), in0=pair(gam_bf, g), in1=pair(rstd, g), op=ALU.mult)
+
+        def shift_of(ob):
+            nc.vector.scalar_tensor_tensor(out=col(shift, ob), in0=col(nmg, ob), scalar=col(rstd, ob), in1=col(bet_bf, ob),
+                                           op0=ALU.mult, op1=ALU.add)
+
         def normalise(ob):
-            n = main.tile([P, NPIX], F32, name="n", tag="z", bufs=3)
+            if ob < 3:
+                n = main.tile([P, NPIX], F32, name="n", tag="z", bufs=3)
+            else:
+                n = main.tile([P, NPIX], F32, name="n_last", tag="ev", bufs=2)
             nc.scalar.activation(out=n[:].rearrange("p (b y x) -> p b y x", b=NB, x=16),
                                  in_=att[:, ob, :].rearrange("p (y b x) -> p b y x", b=NB, x=16),
-                                 func=ACT.Identity, bias=shift[:, ob:ob + 1], scale=gain[:, ob:ob + 1])
+                                 func=ACT.Identity, bias=col(shift, ob), scale=col(gain, ob))
             ns[ob] = n
 
         def negative_part(ob):
-            neg = main.tile([P, NPIX], F32, name="neg", tag="ev", bufs=2)
+            neg = main.tile([P, NPIX], F32, name="neg", tag=("t1", "t2")[ob % 2], bufs=1)
             nc.vector.tensor_scalar(out=neg[:], in0=ns[ob][:], scalar1=0.0, scalar2=a_col[:, 0:1],
                                     op0=ALU.min, op1=ALU.mult)
             negs[ob] = neg
@@ -556,12 +590,51 @@ def tile_merge_pa_kernel(tc, x, w_c1, b_c1, w_q, w_k, w_v, bn_gamma, bn_beta, pr
                                            op0=ALU.max, op1=ALU.add)
             nc.sync.dma_start(out=out_v[:, ob], in_=res[:].rearrange("p (b f) -> p b f", b=NB))
 
+        B6 = STEPS - 2
+        B7 = STEPS - 1
+        divide_block(B6, 0)
+        divide_block(B7, 0)
+        last_squares(0)
+        divide_block(B6, 1)
+        last_sum(0)
+        divide_block(B7, 1)
+        last_squares(1)
+        divide_block(B6, 2)
+        last_sum(1)
+        totals(0)
+        divide_block(B7, 2)
+        last_squares(2)
+        mean_squared(0)
+        minus_mean(0)
+        var_plus_eps(0)
+        std(0)
+        minus_mean_gamma(0)
+        last_sum(2)
+        gain_of(0)
+        shift_of(0)
+        shift_of(1)
         normalise(0)
+        divide_block(B6, 3)
+        divide_block(B7, 3)
+        last_squares(3)
         normalise(1)
+        last_sum(3)
         negative_part(0)
-        for ob in range(4):
-            if ob + 2 < 4:
-                normalise(ob + 2)
-            if ob + 1 < 4:
-                negative_part(ob + 1)
-            prelu_and_store(ob)
+        totals(1)
+        mean_squared(1)
+        minus_mean(1)
+        var_plus_eps(1)
+        std(1)
+        minus_mean_gamma(1)
+        gain_of(1)
+        shift_of(2)
+        shift_of(3)
+        normalise(2)
+        normalise(3)
+        prelu_and_store(0)
+        negative_part(1)
+        negative_part(2)
+        prelu_and_store(1)
+        negative_part(3)
+        prelu_and_store(2)
+        prelu_and_store(3)

@@ -129,6 +129,7 @@ def tile_merge_pa_kernel(tc, x, w_c1, b_c1, w_q, w_k, w_v, bn_gamma, bn_beta, pr
         rds = {}
         lgs = {}
         banks = {}
+        ev_sums = []
 
         def ok(s):
             return 0 <= s < STEPS
@@ -212,6 +213,13 @@ def tile_merge_pa_kernel(tc, x, w_c1, b_c1, w_q, w_k, w_v, bn_gamma, bn_beta, pr
                         den = psm.tile([P, 4, P], F32, name="den", tag="den", bufs=1)
                     dens[s] = den
                 add_up(dens[s], zs[s], j)
+            elif kind == "G" and s == STEPS - 2:
+                if j == 0:
+                    num = psm.tile([P, 4, P], F32, name="num", tag="num", bufs=1)
+                    nums[s] = num
+                ob = j // 3
+                nc.tensor.matmul(out=nums[s][:, ob, :], lhsT=ev_sums[0][:, j % 3, P * ob:P * (ob + 1)], rhs=ident[:],
+                                 is_transpose=True, start=(j % 3 == 0), stop=(j % 3 == 2))
             else:
                 if j == 0:
                     if s == STEPS - 1:
@@ -257,8 +265,8 @@ def tile_merge_pa_kernel(tc, x, w_c1, b_c1, w_q, w_k, w_v, bn_gamma, bn_beta, pr
             if ok(s - 2) and s - 2 < STEPS - 2:
                 pe_list.extend([("G", s - 2, i) for i in range(36)])
         for ob in range(4):
-            for s in (STEPS - 2, STEPS - 1):
-                pe_list.extend([("G", s, 9 * ob + j) for j in range(9)])
+            pe_list.extend([("G", STEPS - 2, 3 * ob + j) for j in range(3)])
+            pe_list.extend([("G", STEPS - 1, 9 * ob + j) for j in range(9)])
 
         done = set()
         pos = [0]
@@ -497,13 +505,19 @@ def tile_merge_pa_kernel(tc, x, w_c1, b_c1, w_q, w_k, w_v, bn_gamma, bn_beta, pr
         divide(STEPS - 3)
         exps(STEPS - 1, 0)
         moments(STEPS - 3)
-        weigh(STEPS - 2, 0, 9)
+        weigh(STEPS - 2, 0, 6)
+        ev_sum = main.tile([P, 3, 512], F32, name="ev_sum", tag="t1", bufs=1)
+        ev_sums.append(ev_sum)
+        ev6 = evs[STEPS - 2]
+        nc.gpsimd.tensor_tensor(out=ev_sum[:], in0=ev6[:, 0:3, :], in1=ev6[:, 3:6, :], op=ALU.add)
+        weigh(STEPS - 2, 6, 9)
+        nc.gpsimd.tensor_tensor(out=ev_sum[:], in0=ev_sum[:], in1=ev6[:, 6:9, :], op=ALU.add)
         exps(STEPS - 1, 1)
         exps(STEPS - 1, 2)
         weigh(STEPS - 1, 0, 9)
         log_den(STEPS - 2)
-        log_den(STEPS - 1)
         exp_minus_log(STEPS - 2)
+        log_den(STEPS - 1)
         exp_minus_log(STEPS - 1)
 
         last = slice(P * (STEPS - 2), NPIX)
@@ -523,7 +537,7 @@ def tile_merge_pa_kernel(tc, x, w_c1, b_c1, w_q, w_k, w_v, bn_gamma, bn_beta, pr
             return t[:, ob:ob + 1]
 
         def divide_block(s, ob):
-            pump_to(("G", s, 9 * ob + 8))
+            pump_to(("G", s, 3 * ob + 2 if s == STEPS - 2 else 9 * ob + 8))
             nc.vector.tensor_tensor(out=att[:, ob, P * s:P * (s + 1)], in0=nums[s][:, ob, :], in1=rds[s][:, ob, :], op=ALU.mult)
 
         def last_sum(ob):

@@ -19,7 +19,8 @@ STEPS = 8
 BN_EPS = 1e-5
 BANK_DT = BF16
 AHEAD = 3
-T_BURST = 6
+MX_RUN = 3
+T_BURST = 9
 LAST_ON_VECTOR = 3
 PIECES = ((0, 4), (4, 4), (8, 8))
 HAAR_ON_VECTOR = ((0, 0), (0, 1), (1, 2), (1, 3), (2, 0), (2, 1), (2, 2))
@@ -254,7 +255,7 @@ def tile_merge_pa_kernel(tc, x, w_c1, b_c1, w_q, w_k, w_v, bn_gamma, bn_beta, pr
                 sums = []
             for n, tok in enumerate(mms):
                 pe_list.append(tok)
-                if n % 2 == 1:
+                if n % MX_RUN == MX_RUN - 1:
                     pe_list.extend(sums[:T_BURST])
                     sums = sums[T_BURST:]
             pe_list.extend(sums)

@@ -98,9 +98,10 @@ def tile_merge_pa_kernel(tc, x, w_c1, b_c1, w_q, w_k, w_v, bn_gamma, bn_beta, pr
             y_scales.append(yst)
 
         att = keep.tile([P, 4, NPIX], F32, name="att")
-        msums = keep.tile([P, 2, 4, STEPS], F32, name="msums")
-        nc.vector.memset(msums[:, :, :, STEPS - 1], 0.0)
-        nc.vector.tensor_scalar(out=msums[:, 1, :, STEPS - 1], in0=msums[:, 1, :, STEPS - 1], scalar1=NPIX * BN_EPS,
+        PAIRS = STEPS // 2
+        msums = keep.tile([P, 2, 4, PAIRS + 1], F32, name="msums")
+        nc.vector.memset(msums[:, :, :, PAIRS], 0.0)
+        nc.vector.tensor_scalar(out=msums[:, 1, :, PAIRS], in0=msums[:, 1, :, PAIRS], scalar1=NPIX * BN_EPS,
                                 scalar2=None, op0=ALU.add)
         neg_pivot = keep.tile([P, 4], F32, name="neg_pivot")
         a_col = keep.tile([P, 1], F32, name="a_col")
@@ -420,21 +421,14 @@ def tile_merge_pa_kernel(tc, x, w_c1, b_c1, w_q, w_k, w_v, bn_gamma, bn_beta, pr
                 nc.vector.tensor_scalar(out=neg_pivot[:], in0=att[:, :, 0], scalar1=-1.0, scalar2=None,
                                         op0=ALU.mult)
 
-        def moments(s, sums_on_vector=False):
-            cols = slice(P * s, P * (s + 1))
+        def moments(s):
+            cols = slice(P * s, P * (s + 2))
             for ob in range(4):
-                if sums_on_vector:
-                    junk_v = main.tile([P, P], F32, name="junk_v", tag="junk_v")
-                    nc.vector.tensor_scalar(out=junk_v[:], in0=att[:, ob, cols], scalar1=neg_pivot[:, ob:ob + 1],
-                                            scalar2=None, op0=ALU.add, op1=ALU.add,
-                                            accum_out=msums[:, 0, ob, s:s + 1])
                 for kind, func in enumerate((ACT.Identity, ACT.Square)):
-                    if kind == 0 and sums_on_vector:
-                        continue
-                    junk = main.tile([P, P], F32, name="junk", tag="junk")
+                    junk = main.tile([P, 2 * P], F32, name="junk", tag="junk")
                     nc.scalar.activation(out=junk[:], in_=att[:, ob, cols], func=func,
                                          bias=neg_pivot[:, ob:ob + 1], scale=1.0,
-                                         accum_out=msums[:, kind, ob, s:s + 1])
+                                         accum_out=msums[:, kind, ob, s // 2:s // 2 + 1])
 
         nc.vector.memset(zeros_bf[:], 0.0)
         g_c1 = weight_copies(W_C1)
@@ -492,8 +486,6 @@ def tile_merge_pa_kernel(tc, x, w_c1, b_c1, w_q, w_k, w_v, bn_gamma, bn_beta, pr
                 haar_from_pe(2)
                 quant_y(1)
                 scores(1, 0, AHEAD)
-            if ok(s - 3):
-                moments(s - 3)
             if ok(s - 1):
                 exps(s - 1, 1)
             if ok(s - 1):
@@ -503,9 +495,10 @@ def tile_merge_pa_kernel(tc, x, w_c1, b_c1, w_q, w_k, w_v, bn_gamma, bn_beta, pr
                 shift_copies(2, False)
             if ok(s - 2):
                 one_over_den(s - 2)
+            if ok(s - 3) and (s - 3) % 2 == 1:
+                moments(s - 4)
         divide(STEPS - 3)
         exps(STEPS - 1, 0)
-        moments(STEPS - 3)
         weigh(STEPS - 2, 0, 6)
         ev_sum = main.tile([P, 3, 512], F32, name="ev_sum", tag="t1", bufs=1)
         ev_sums.append(ev_sum)
@@ -515,6 +508,7 @@ def tile_merge_pa_kernel(tc, x, w_c1, b_c1, w_q, w_k, w_v, bn_gamma, bn_beta, pr
         nc.gpsimd.tensor_tensor(out=ev_sum[:], in0=ev_sum[:], in1=ev6[:, 6:9, :], op=ALU.add)
         exps(STEPS - 1, 1)
         exps(STEPS - 1, 2)
+        moments(STEPS - 4)
         weigh(STEPS - 1, 0, 9)
         log_den(STEPS - 2)
         exp_minus_log(STEPS - 2)
@@ -544,12 +538,12 @@ def tile_merge_pa_kernel(tc, x, w_c1, b_c1, w_q, w_k, w_v, bn_gamma, bn_beta, pr
         def last_sum(ob):
             junk_v = main.tile([P, 2 * P], F32, name="junk_v", tag="junk_v")
             nc.vector.tensor_scalar(out=junk_v[:], in0=att[:, ob, last], scalar1=col(neg_pivot, ob), scalar2=None,
-                                    op0=ALU.add, op1=ALU.add, accum_out=msums[:, 0, ob, STEPS - 2:STEPS - 1])
+                                    op0=ALU.add, op1=ALU.add, accum_out=msums[:, 0, ob, PAIRS - 1:PAIRS])
 
         def last_squares(ob):
             junk = main.tile([P, 2 * P], F32, name="junk2", tag="junk2")
             nc.scalar.activation(out=junk[:], in_=att[:, ob, last], func=ACT.Square, bias=col(neg_pivot, ob), scale=1.0,
-                                 accum_out=msums[:, 1, ob, STEPS - 2:STEPS - 1])
+                                 accum_out=msums[:, 1, ob, PAIRS - 1:PAIRS])
 
         def pair(t, g):
             return t[:, 2 * g:2 * g + 2]

@@ -19,12 +19,16 @@ STEPS = 8
 BN_EPS = 1e-5
 BANK_DT = BF16
 AHEAD = 3
-MX_RUN = 3
-T_BURST = 9
+SHARE_FROM = 1
+LATE = 2
 LAST_ON_VECTOR = 3
 PIECES = ((0, 4), (4, 4), (8, 8))
 HAAR_ON_VECTOR = ((0, 0), (0, 1), (1, 2), (1, 3), (2, 0), (2, 1), (2, 2))
-W_C1, W_K, W_Q, W_V = 0, 1, 2, 3
+W_C1, W_K, W_Q, W_V, W_KN = 0, 1, 2, 3, 4
+CENTRE = 4
+AROUND = (0, 1, 2, 3, 5, 6, 7, 8)
+OFFSET_OF_SLOT = AROUND + (CENTRE,)
+GROUPS = ((0, 3), (3, 6), (6, 8))
 
 FLOPS = 4 * 2 * 512 * 512 * 1024
 
@@ -79,7 +83,7 @@ def tile_merge_pa_kernel(tc, x, w_c1, b_c1, w_q, w_k, w_v, bn_gamma, bn_beta, pr
 
         w_codes = []
         w_scales = []
-        for i in range(4):
+        for i in range(5):
             wct = keep.tile([P, 512], I32, name="w_codes%d" % i, align_bytes=64)
             wst = keep.tile([P, 512], U8, name="w_scales%d" % i, align_bytes=64)
             w_codes.append(wct)
@@ -130,19 +134,22 @@ def tile_merge_pa_kernel(tc, x, w_c1, b_c1, w_q, w_k, w_v, bn_gamma, bn_beta, pr
         q_sbs = {}
         rds = {}
         lgs = {}
+        ms = {}
         banks = {}
         ev_sums = []
 
         def ok(s):
             return 0 <= s < STEPS
 
-        def conv(dst, s, j, wi):
-            c0 = ROW + P * s + ROW * (j // 3 - 1)
-            d = j % 3
+        def conv(dst, s, j, wi, start=True, stop=True):
+            window(dst, 2 * s + j // 3 - 1, j % 3, wi, start, stop)
+
+        def window(dst, r, d, wi, start=True, stop=True):
+            c0 = ROW + ROW * r
             nc.tensor.matmul_mx(out=dst, lhsT=y_codes[d][:, c0:c0 + P].bitcast(FP8X4),
                                 lhsT_scale=y_scales[d][:, c0:c0 + P],
                                 rhs=w_codes[wi][:].bitcast(FP8X4), rhs_scale=w_scales[wi][:],
-                                start=True, stop=True)
+                                start=start, stop=stop)
 
         def first_conv(bank, r):
             cols = slice(P * r, P * (r + 1))
@@ -167,11 +174,12 @@ def tile_merge_pa_kernel(tc, x, w_c1, b_c1, w_q, w_k, w_v, bn_gamma, bn_beta, pr
                 banks[tok] = q_ps
             elif kind == "k":
                 k_ps = psm.tile([P, 512], F32, name="k_ps", tag="k_ps", bufs=3)
-                conv(k_ps[:], s, j, W_K)
+                conv(k_ps[:], s, AROUND[j], W_K, True, False)
+                conv(k_ps[:], s, CENTRE, W_KN, False, True)
                 banks[tok] = k_ps
-            elif kind == "v":
+            elif kind in ("v", "u"):
                 v_ps = psm.tile([P, 512], F32, name="v_ps", tag="v_ps", bufs=3)
-                conv(v_ps[:], s, j, W_V)
+                window(v_ps[:], s, j, W_V)
                 banks[tok] = v_ps
             elif kind == "c":
                 bank = psm.tile([P, 4, P], BANK_DT, name="bank", tag="v_ps", bufs=3)
@@ -231,6 +239,26 @@ def tile_merge_pa_kernel(tc, x, w_c1, b_c1, w_q, w_k, w_v, bn_gamma, bn_beta, pr
                     nums[s] = num
                 add_up(nums[s], evs[s], j)
 
+        def products(a):
+            todo = []
+            if a <= SHARE_FROM:
+                todo.extend([(("u", 2 * a - 1, d), a, d) for d in range(3)])
+            todo.append((("v", 2 * a, 0), a, 3))
+            todo.append((("v", 2 * a, 2), a, 4))
+            for d in range(3):
+                todo.append((("v", 2 * a + 1, d), a, 5 + d))
+                if ok(a + 1) and a >= SHARE_FROM:
+                    todo.append((("v", 2 * a + 1, d), a + 1, d))
+            todo.append((("v", 2 * a, 1), a, 8))
+            return todo
+
+        def v_banks(a):
+            toks = []
+            for tok, s, slot in products(a):
+                if tok not in toks:
+                    toks.append(tok)
+            return toks
+
         def on_pe(pc):
             return [("h", pc, b) for b in range(NB) if (pc, b) not in HAAR_ON_VECTOR]
 
@@ -238,34 +266,38 @@ def tile_merge_pa_kernel(tc, x, w_c1, b_c1, w_q, w_k, w_v, bn_gamma, bn_beta, pr
                                                                  ("w", W_K, 0), ("w", W_K, 1)] + on_pe(1)
         pe_list += [("q", 0, 0)] + [("k", 0, j) for j in range(AHEAD)]
         for s in range(STEPS + 2):
-            mms = []
+            a = s - 2
             if ok(s):
-                mms.extend([("k", s, j) for j in range(AHEAD, 9)])
+                pe_list.extend([("k", s, j) for j in range(AHEAD if s == 0 else AHEAD + LATE, 8)])
             if ok(s + 1):
-                mms.append(("q", s + 1, 0))
+                pe_list.append(("q", s + 1, 0))
             if s == 0:
-                mms.extend([("C", 1, t) for t in range(4)] + [("w", W_V, 0), ("w", W_V, 1)] + on_pe(2))
+                pe_list.extend([("C", 1, t) for t in range(4)] + [("w", W_V, 0), ("w", W_V, 1)] + on_pe(2))
             if s == 1:
-                mms.extend([("C", 2, t) for t in range(4)])
-            sums = []
-            if ok(s - 2):
-                mms.extend([("v", s - 2, j) for j in range(0 if s == 2 else AHEAD, 9)])
-                sums = [("F", s - 2, i) for i in range(36)]
-            if s == STEPS:
-                pe_list.extend(sums)
-                sums = []
-            for n, tok in enumerate(mms):
-                pe_list.append(tok)
-                if n % MX_RUN == MX_RUN - 1:
-                    pe_list.extend(sums[:T_BURST])
-                    sums = sums[T_BURST:]
-            pe_list.extend(sums)
+                pe_list.extend([("C", 2, t) for t in range(4)])
+            vb = v_banks(a) if ok(a) else []
+            den_sums = [("F", a, i) for i in range(36)] if ok(a) else []
+            num_sums = [("G", a, i) for i in range(36)] if ok(a) and a < STEPS - 2 else []
+            if a == STEPS - 2:
+                pe_list.extend(den_sums)
+                den_sums = []
+            if a == STEPS - 1:
+                pe_list.extend(vb)
+                vb = []
+            pe_list.extend(vb[:3])
+            pe_list.extend(den_sums[:9])
+            pe_list.extend(vb[3:5])
+            pe_list.extend(den_sums[9:18])
+            pe_list.extend(vb[5:])
             if ok(s + 1):
                 pe_list.extend([("k", s + 1, j) for j in range(AHEAD)])
-            if ok(s - 1) and s != 1:
-                pe_list.extend([("v", s - 1, j) for j in range(AHEAD)])
-            if ok(s - 2) and s - 2 < STEPS - 2:
-                pe_list.extend([("G", s - 2, i) for i in range(36)])
+            pe_list.extend(den_sums[18:])
+            pe_list.extend(num_sums[:27])
+            if ok(s + 1):
+                pe_list.append(("k", s + 1, AHEAD))
+            pe_list.extend(num_sums[27:])
+            if ok(s + 1):
+                pe_list.append(("k", s + 1, AHEAD + 1))
         for ob in range(4):
             pe_list.extend([("G", STEPS - 2, 3 * ob + j) for j in range(3)])
             pe_list.extend([("G", STEPS - 1, 9 * ob + j) for j in range(9)])
@@ -375,28 +407,29 @@ def tile_merge_pa_kernel(tc, x, w_c1, b_c1, w_q, w_k, w_v, bn_gamma, bn_beta, pr
             t2 = main.tile([P, 2, 512], F32, name="t2", tag="t2", bufs=1)
             nc.vector.tensor_tensor(out=t2[:], in0=t1[:, 0:2, :], in1=t1[:, 2:4, :], op=ALU.max)
             between[1]()
-            t3 = main.tile([P, 512], F32, name="t3", tag="t3", bufs=1)
-            nc.vector.tensor_tensor(out=t3[:], in0=t2[:, 0, :], in1=t2[:, 1, :], op=ALU.max)
-            between[2]()
             m = main.tile([P, 512], F32, name="m", tag="m")
-            nc.vector.tensor_tensor(out=m[:], in0=t3[:], in1=z[:, 8, :], op=ALU.max)
-            m_thrice = m[:].unsqueeze(1).to_broadcast([P, 3, 512])
-            for g in range(3):
+            nc.vector.scalar_tensor_tensor(out=m[:], in0=t2[:, 0, :], scalar=0.0, in1=t2[:, 1, :], op0=ALU.max, op1=ALU.max)
+            ms[s] = m
+            between[2]()
+            for g, (g0, g1) in enumerate(GROUPS):
                 eng = nc.vector if 3 * g < on_vector else nc.gpsimd
-                eng.tensor_tensor(out=z[:, 3 * g:3 * g + 3, :], in0=z[:, 3 * g:3 * g + 3, :], in1=m_thrice, op=ALU.subtract)
+                eng.tensor_tensor(out=z[:, g0:g1, :], in0=z[:, g0:g1, :], in1=m[:].unsqueeze(1).to_broadcast([P, g1 - g0, 512]),
+                                  op=ALU.subtract)
 
         def exps(s, g):
             z = zs[s]
-            nc.scalar.activation(out=z[:, 3 * g:3 * g + 3, :], in_=z[:, 3 * g:3 * g + 3, :], func=ACT.Exp)
+            if g == 0:
+                nc.scalar.activation(out=z[:, 8, :], in_=ms[s][:], func=ACT.Exp, scale=-1.0)
+            g0, g1 = GROUPS[g]
+            nc.scalar.activation(out=z[:, g0:g1, :], in_=z[:, g0:g1, :], func=ACT.Exp)
 
-        def weigh(s, j0, j1):
-            if j0 == 0:
-                ev = main.tile([P, 9, 512], F32, name="ev", tag="ev", bufs=2)
-                evs[s] = ev
-            for j in range(j0, j1):
-                pump_to(("v", s, j))
-                nc.vector.tensor_tensor(out=evs[s][:, j, :], in0=zs[s][:, j, :], in1=banks[("v", s, j)][:],
-                                        op=ALU.mult)
+        def weigh(a, i0, i1):
+            for tok, s, slot in products(a)[i0:i1]:
+                pump_to(tok)
+                if s not in evs:
+                    ev = main.tile([P, 9, 512], F32, name="ev", tag="ev", bufs=2)
+                    evs[s] = ev
+                nc.vector.tensor_tensor(out=evs[s][:, slot, :], in0=zs[s][:, slot, :], in1=banks[tok][:], op=ALU.mult)
 
         def log_den(s):
             pump_to(("F", s, 35))
@@ -446,7 +479,10 @@ def tile_merge_pa_kernel(tc, x, w_c1, b_c1, w_q, w_k, w_v, bn_gamma, bn_beta, pr
         shift_copies(0, True)
         g_k = weight_copies(W_K)
         quant_y(0)
+        g_kn = main.tile([P, 2048], BF16, name="grouped_neg", tag="grouped", bufs=2, align_bytes=64)
+        nc.vector.tensor_scalar(out=g_kn[:], in0=g_k[:], scalar1=-1.0, scalar2=None, op0=ALU.mult)
         quant_w(W_K, g_k)
+        quant_w(W_KN, g_kn)
         q_copy(0)
         haar_from_pe(1)
 
@@ -458,7 +494,7 @@ def tile_merge_pa_kernel(tc, x, w_c1, b_c1, w_q, w_k, w_v, bn_gamma, bn_beta, pr
 
         scores(0, 0, AHEAD)
         for s in range(STEPS):
-            scores(s, AHEAD, 9)
+            scores(s, AHEAD, 8)
             if s == 0:
                 haar_on_vector(1, (2, 3))
             if ok(s - 1):
@@ -468,7 +504,7 @@ def tile_merge_pa_kernel(tc, x, w_c1, b_c1, w_q, w_k, w_v, bn_gamma, bn_beta, pr
             if ok(s - 3):
                 divide(s - 3)
             if ok(s - 2):
-                weigh(s - 2, 0, 9)
+                weigh(s - 2, 0, 12)
             if s == 2:
                 quant_y(2)
             if s == 0:
@@ -499,12 +535,12 @@ def tile_merge_pa_kernel(tc, x, w_c1, b_c1, w_q, w_k, w_v, bn_gamma, bn_beta, pr
                 moments(s - 4)
         divide(STEPS - 3)
         exps(STEPS - 1, 0)
-        weigh(STEPS - 2, 0, 6)
+        weigh(STEPS - 2, 0, 3)
         ev_sum = main.tile([P, 3, 512], F32, name="ev_sum", tag="t1", bufs=1)
         ev_sums.append(ev_sum)
         ev6 = evs[STEPS - 2]
         nc.gpsimd.tensor_tensor(out=ev_sum[:], in0=ev6[:, 0:3, :], in1=ev6[:, 3:6, :], op=ALU.add)
-        weigh(STEPS - 2, 6, 9)
+        weigh(STEPS - 2, 3, 9)
         nc.gpsimd.tensor_tensor(out=ev_sum[:], in0=ev_sum[:], in1=ev6[:, 6:9, :], op=ALU.add)
         exps(STEPS - 1, 1)
         exps(STEPS - 1, 2)

@@ -399,7 +399,7 @@ def tile_merge_pa_kernel(tc, x, w_c1, b_c1, w_q, w_k, w_v, bn_gamma, bn_beta, pr
                     zs[s] = z
                 nc.vector.tensor_tensor(out=zs[s][:, j, :], in0=q_sbs[s][:], in1=banks[("k", s, j)][:], op=ALU.mult)
 
-        def shift_by_max(s, between, on_vector=0):
+        def shift_by_max(s, between, on_vector=0, all_before_m=False):
             z = zs[s]
             t1 = main.tile([P, 4, 512], F32, name="t1", tag="t1", bufs=1)
             nc.vector.tensor_tensor(out=t1[:], in0=z[:, 0:4, :], in1=z[:, 4:8, :], op=ALU.max)
@@ -407,10 +407,13 @@ def tile_merge_pa_kernel(tc, x, w_c1, b_c1, w_q, w_k, w_v, bn_gamma, bn_beta, pr
             t2 = main.tile([P, 2, 512], F32, name="t2", tag="t2", bufs=1)
             nc.vector.tensor_tensor(out=t2[:], in0=t1[:, 0:2, :], in1=t1[:, 2:4, :], op=ALU.max)
             between[1]()
+            if all_before_m:
+                between[2]()
             m = main.tile([P, 512], F32, name="m", tag="m")
             nc.vector.scalar_tensor_tensor(out=m[:], in0=t2[:, 0, :], scalar=0.0, in1=t2[:, 1, :], op0=ALU.max, op1=ALU.max)
             ms[s] = m
-            between[2]()
+            if not all_before_m:
+                between[2]()
             for g, (g0, g1) in enumerate(GROUPS):
                 eng = nc.vector if 3 * g < on_vector else nc.gpsimd
                 eng.tensor_tensor(out=z[:, g0:g1, :], in0=z[:, g0:g1, :], in1=m[:].unsqueeze(1).to_broadcast([P, g1 - g0, 512]),
@@ -450,9 +453,6 @@ def tile_merge_pa_kernel(tc, x, w_c1, b_c1, w_q, w_k, w_v, bn_gamma, bn_beta, pr
             pump_to(("G", s, 35))
             cols = slice(P * s, P * (s + 1))
             nc.vector.tensor_tensor(out=att[:, :, cols], in0=nums[s][:], in1=rds[s][:], op=ALU.mult)
-            if s == 0:
-                nc.vector.tensor_scalar(out=neg_pivot[:], in0=att[:, :, 0], scalar1=-1.0, scalar2=None,
-                                        op0=ALU.mult)
 
         def moments(s):
             cols = slice(P * s, P * (s + 2))
@@ -509,10 +509,10 @@ def tile_merge_pa_kernel(tc, x, w_c1, b_c1, w_q, w_k, w_v, bn_gamma, bn_beta, pr
                 quant_y(2)
             if s == 0:
                 shift_by_max(s, (lambda: (quant_ll(1), q_copy(1), add_bias_on_scalar(1), shift_copies(1, False)),
-                                 lambda: haar_on_vector(2, (0, 1)), lambda: haar_on_vector(2, (2,))))
+                                 lambda: haar_on_vector(2, (0, 1)), lambda: (haar_on_vector(2, (2,)), quant_y(1))), 0, True)
             elif s == 1:
                 shift_by_max(s, (lambda: quant_ll(2), lambda: quant_w(W_V, g_v),
-                                 lambda: nc.vector.tensor_copy(out=a_col[:], in_=a_bf[:])))
+                                 lambda: nc.vector.tensor_copy(out=a_col[:], in_=a_bf[:])), 0, True)
                 scores(s + 1, 0, AHEAD)
             else:
                 shift_by_max(s, (early_scores(s + 1, 0), early_scores(s + 1, 1), early_scores(s + 1, 2)),
@@ -520,7 +520,6 @@ def tile_merge_pa_kernel(tc, x, w_c1, b_c1, w_q, w_k, w_v, bn_gamma, bn_beta, pr
             if s == 0:
                 g_v = weight_copies(W_V)
                 haar_from_pe(2)
-                quant_y(1)
                 scores(1, 0, AHEAD)
             if ok(s - 1):
                 exps(s - 1, 1)
@@ -531,6 +530,8 @@ def tile_merge_pa_kernel(tc, x, w_c1, b_c1, w_q, w_k, w_v, bn_gamma, bn_beta, pr
                 shift_copies(2, False)
             if ok(s - 2):
                 one_over_den(s - 2)
+            if s == 3:
+                nc.scalar.activation(out=neg_pivot[:], in_=att[:, :, 0], func=ACT.Copy, scale=-1.0)
             if ok(s - 3) and (s - 3) % 2 == 1:
                 moments(s - 4)
         divide(STEPS - 3)

@@ -109,7 +109,6 @@ def tile_merge_pa_kernel(tc, x, w_c1, b_c1, w_q, w_k, w_v, bn_gamma, bn_beta, pr
                                 scalar2=None, op0=ALU.add)
         neg_pivot = keep.tile([P, 4], F32, name="neg_pivot")
         a_col = keep.tile([P, 1], F32, name="a_col")
-        zeros_bf = keep.tile([P, P], BF16, name="zeros_bf")
         bias_full = keep.tile([P, P, 4], BF16, name="bias_full")
 
         ll = mid.tile([P, NPIX, 4], BF16, name="ll", align_bytes=64)
@@ -182,7 +181,10 @@ def tile_merge_pa_kernel(tc, x, w_c1, b_c1, w_q, w_k, w_v, bn_gamma, bn_beta, pr
                 window(v_ps[:], s, j, W_V)
                 banks[tok] = v_ps
             elif kind == "c":
-                bank = psm.tile([P, 4, P], BANK_DT, name="bank", tag="v_ps", bufs=3)
+                if s == STEPS - 1:
+                    bank = psm.tile([P, 4, P], BANK_DT, name="bank_last", tag="num", bufs=1)
+                else:
+                    bank = psm.tile([P, 4, P], BANK_DT, name="bank", tag="v_ps", bufs=3)
                 first_conv(bank, s)
                 banks[tok] = bank
             elif kind == "C":
@@ -274,7 +276,7 @@ def tile_merge_pa_kernel(tc, x, w_c1, b_c1, w_q, w_k, w_v, bn_gamma, bn_beta, pr
             if s == 0:
                 pe_list.extend([("C", 1, t) for t in range(4)] + [("w", W_V, 0), ("w", W_V, 1)] + on_pe(2))
             if s == 1:
-                pe_list.extend([("C", 2, t) for t in range(4)])
+                pe_list.extend([("c", r, 0) for r in range(4, 8)])
             vb = v_banks(a) if ok(a) else []
             den_sums = [("F", a, i) for i in range(36)] if ok(a) else []
             num_sums = [("G", a, i) for i in range(36)] if ok(a) and a < STEPS - 2 else []
@@ -463,13 +465,10 @@ def tile_merge_pa_kernel(tc, x, w_c1, b_c1, w_q, w_k, w_v, bn_gamma, bn_beta, pr
                                          bias=neg_pivot[:, ob:ob + 1], scale=1.0,
                                          accum_out=msums[:, kind, ob, s // 2:s // 2 + 1])
 
-        nc.vector.memset(zeros_bf[:], 0.0)
         g_c1 = weight_copies(W_C1)
         haar_on_vector(0, (0, 1))
         quant_w(W_C1, g_c1)
-        for t in range(4):
-            nc.vector.tensor_scalar(out=bias_full[:, :, t], in0=zeros_bf[:], scalar1=bias_bf[:, t:t + 1],
-                                    scalar2=None, op0=ALU.add)
+        nc.vector.tensor_copy(out=bias_full[:], in_=bias_bf[:].unsqueeze(1).to_broadcast([P, P, 4]))
         haar_from_pe(0)
         quant_ll(0)
         g_q = weight_copies(W_Q)
@@ -513,6 +512,8 @@ def tile_merge_pa_kernel(tc, x, w_c1, b_c1, w_q, w_k, w_v, bn_gamma, bn_beta, pr
             elif s == 1:
                 shift_by_max(s, (lambda: quant_ll(2), lambda: quant_w(W_V, g_v),
                                  lambda: nc.vector.tensor_copy(out=a_col[:], in_=a_bf[:])), 0, True)
+                for r in range(4, 8):
+                    add_bias(r)
                 scores(s + 1, 0, AHEAD)
             else:
                 shift_by_max(s, (early_scores(s + 1, 0), early_scores(s + 1, 1), early_scores(s + 1, 2)),
@@ -526,7 +527,6 @@ def tile_merge_pa_kernel(tc, x, w_c1, b_c1, w_q, w_k, w_v, bn_gamma, bn_beta, pr
             if ok(s - 1):
                 exps(s - 1, 2)
             if s == 1:
-                add_bias_on_scalar(2)
                 shift_copies(2, False)
             if ok(s - 2):
                 one_over_den(s - 2)

@@ -108,7 +108,8 @@ def tile_merge_pa_kernel(tc, x, w_c1, b_c1, w_q, w_k, w_v, bn_gamma, bn_beta, pr
         nc.vector.tensor_scalar(out=msums[:, 1, :, PAIRS], in0=msums[:, 1, :, PAIRS], scalar1=NPIX * BN_EPS,
                                 scalar2=None, op0=ALU.add)
         neg_pivot = keep.tile([P, 4], F32, name="neg_pivot")
-        a_col = keep.tile([P, 1], F32, name="a_col")
+        one_minus_a = keep.tile([P, 1], F32, name="one_minus_a")
+        gam_f = keep.tile([P, 4], F32, name="gam_f")
         bias_full = keep.tile([P, P, 4], BF16, name="bias_full")
 
         ll = mid.tile([P, NPIX, 4], BF16, name="ll", align_bytes=64)
@@ -336,18 +337,22 @@ def tile_merge_pa_kernel(tc, x, w_c1, b_c1, w_q, w_k, w_v, bn_gamma, bn_beta, pr
                 pump_to(tok)
                 halve(pc, tok[2], banks[tok][:, 0:ROW * PIECES[pc][1]])
 
-        def haar_on_vector(pc, images):
+        def haar_on_vector(pc, images, on_gpsimd=False):
+            eng = nc.gpsimd if on_gpsimd else nc.vector
             nr = PIECES[pc][1]
             row_sums = []
             for b in images:
                 rows = x_piece(pc, b).rearrange("p j (i a w) -> p j i a w", a=2, w=32)
-                s1 = main.tile([P, 4, nr, 32], F32, name="s1", tag="s1", bufs=2)
-                nc.vector.tensor_tensor(out=s1[:], in0=rows[:, :, :, 0, :], in1=rows[:, :, :, 1, :], op=ALU.add)
+                if on_gpsimd:
+                    s1 = main.tile([P, 4, nr, 32], F32, name="s1_late", tag="grouped", bufs=2, align_bytes=64)
+                else:
+                    s1 = main.tile([P, 4, nr, 32], F32, name="s1", tag="s1", bufs=2)
+                eng.tensor_tensor(out=s1[:], in0=rows[:, :, :, 0, :], in1=rows[:, :, :, 1, :], op=ALU.add)
                 row_sums.append(s1)
             for b, s1 in zip(images, row_sums):
                 pairs = s1[:].rearrange("p j i (x e) -> p (j i x) e", e=2)
                 s2 = main.tile([P, ROW * nr], F32, name="s2", tag="s2", bufs=3)
-                nc.vector.tensor_tensor(out=s2[:], in0=pairs[:, :, 0], in1=pairs[:, :, 1], op=ALU.add)
+                eng.tensor_tensor(out=s2[:], in0=pairs[:, :, 0], in1=pairs[:, :, 1], op=ALU.add)
                 halve(pc, b, s2[:])
 
         def quant_ll(pc):
@@ -491,11 +496,10 @@ def tile_merge_pa_kernel(tc, x, w_c1, b_c1, w_q, w_k, w_v, bn_gamma, bn_beta, pr
         def early_scores(s, j):
             return (lambda: scores(s, j, j + 1)) if ok(s) else nothing
 
+        haar_on_vector(1, (2, 3), True)
         scores(0, 0, AHEAD)
         for s in range(STEPS):
             scores(s, AHEAD, 8)
-            if s == 0:
-                haar_on_vector(1, (2, 3))
             if ok(s - 1):
                 exps(s - 1, 0)
             if s > 0 and ok(s + 1):
@@ -510,8 +514,7 @@ def tile_merge_pa_kernel(tc, x, w_c1, b_c1, w_q, w_k, w_v, bn_gamma, bn_beta, pr
                 shift_by_max(s, (lambda: (quant_ll(1), q_copy(1), add_bias_on_scalar(1), shift_copies(1, False)),
                                  lambda: haar_on_vector(2, (0, 1)), lambda: (haar_on_vector(2, (2,)), quant_y(1))), 0, True)
             elif s == 1:
-                shift_by_max(s, (lambda: quant_ll(2), lambda: quant_w(W_V, g_v),
-                                 lambda: nc.vector.tensor_copy(out=a_col[:], in_=a_bf[:])), 0, True)
+                shift_by_max(s, (lambda: quant_ll(2), lambda: quant_w(W_V, g_v), nothing), 0, True)
                 for r in range(4, 8):
                     add_bias(r)
                 scores(s + 1, 0, AHEAD)
@@ -532,6 +535,8 @@ def tile_merge_pa_kernel(tc, x, w_c1, b_c1, w_q, w_k, w_v, bn_gamma, bn_beta, pr
                 one_over_den(s - 2)
             if s == 3:
                 nc.scalar.activation(out=neg_pivot[:], in_=att[:, :, 0], func=ACT.Copy, scale=-1.0)
+                nc.scalar.activation(out=one_minus_a[:], in_=a_bf[:], func=ACT.Identity, bias=1.0, scale=-1.0)
+                nc.scalar.copy(out=gam_f[:], in_=gam_bf[:])
             if ok(s - 3) and (s - 3) % 2 == 1:
                 moments(s - 4)
         divide(STEPS - 3)
@@ -555,9 +560,7 @@ def tile_merge_pa_kernel(tc, x, w_c1, b_c1, w_q, w_k, w_v, bn_gamma, bn_beta, pr
         last = slice(P * (STEPS - 2), NPIX)
         tot = keep.tile([P, 2, 4], F32, name="tot")
         dd = keep.tile([P, 4], F32, name="dd")
-        ve = keep.tile([P, 4], F32, name="ve")
         neg_mean = keep.tile([P, 4], F32, name="neg_mean")
-        nmg = keep.tile([P, 4], F32, name="nmg")
         rstd = keep.tile([P, 4], F32, name="rstd")
         gain = keep.tile([P, 4], F32, name="gain")
         shift = keep.tile([P, 4], F32, name="shift")
@@ -582,37 +585,18 @@ def tile_merge_pa_kernel(tc, x, w_c1, b_c1, w_q, w_k, w_v, bn_gamma, bn_beta, pr
             nc.scalar.activation(out=junk[:], in_=att[:, ob, last], func=ACT.Square, bias=col(neg_pivot, ob), scale=1.0,
                                  accum_out=msums[:, 1, ob, PAIRS - 1:PAIRS])
 
-        def pair(t, g):
-            return t[:, 2 * g:2 * g + 2]
+        def totals(ob):
+            nc.vector.tensor_reduce(out=tot[:, :, ob:ob + 1], in_=msums[:, :, ob:ob + 1, :], axis=mybir.AxisListType.X, op=ALU.add)
 
-        def totals(g):
-            nc.vector.tensor_reduce(out=tot[:, :, 2 * g:2 * g + 2], in_=msums[:, :, 2 * g:2 * g + 2, :],
-                                    axis=mybir.AxisListType.X, op=ALU.add)
-
-        def mean_squared(g):
-            nc.vector.scalar_tensor_tensor(out=pair(dd, g), in0=tot[:, 0, 2 * g:2 * g + 2], scalar=1.0 / (NPIX * NPIX),
-                                           in1=tot[:, 0, 2 * g:2 * g + 2], op0=ALU.mult, op1=ALU.mult)
-
-        def var_plus_eps(g):
-            nc.vector.scalar_tensor_tensor(out=pair(ve, g), in0=tot[:, 1, 2 * g:2 * g + 2], scalar=1.0 / NPIX, in1=pair(dd, g),
-                                           op0=ALU.mult, op1=ALU.subtract)
-
-        def std(g):
-            nc.scalar.activation(out=pair(rstd, g), in_=pair(ve, g), func=ACT.Abs_reciprocal_sqrt)
-
-        def minus_mean(g):
-            nc.vector.scalar_tensor_tensor(out=pair(neg_mean, g), in0=tot[:, 0, 2 * g:2 * g + 2], scalar=-1.0 / NPIX,
-                                           in1=pair(neg_pivot, g), op0=ALU.mult, op1=ALU.add)
-
-        def minus_mean_gamma(g):
-            nc.vector.tensor_tensor(out=pair(nmg, g), in0=pair(neg_mean, g), in1=pair(gam_bf, g), op=ALU.mult)
-
-        def gain_of(g):
-            nc.vector.tensor_tensor(out=pair(gain, g), in0=pair(gam_bf, g), in1=pair(rstd, g), op=ALU.mult)
-
-        def shift_of(ob):
-            nc.vector.scalar_tensor_tensor(out=col(shift, ob), in0=col(nmg, ob), scalar=col(rstd, ob), in1=col(bet_bf, ob),
-                                           op0=ALU.mult, op1=ALU.add)
+        def statistics(ob):
+            nc.scalar.activation(out=col(dd, ob), in_=tot[:, 0, ob:ob + 1], func=ACT.Square, scale=1.0 / NPIX)
+            nc.scalar.activation(out=col(neg_mean, ob), in_=tot[:, 0, ob:ob + 1], func=ACT.Identity, bias=col(neg_pivot, ob),
+                                 scale=-1.0 / NPIX)
+            nc.scalar.activation(out=col(rstd, ob), in_=tot[:, 1, ob:ob + 1], func=ACT.Abs_reciprocal_sqrt, bias=col(dd, ob),
+                                 scale=-1.0 / NPIX)
+            nc.scalar.activation(out=col(gain, ob), in_=col(rstd, ob), func=ACT.Copy, scale=col(gam_f, ob))
+            nc.scalar.activation(out=col(shift, ob), in_=col(gain, ob), func=ACT.Identity, bias=col(bet_bf, ob),
+                                 scale=col(neg_mean, ob))
 
         def normalise(ob):
             if ob < 3:
@@ -624,16 +608,18 @@ def tile_merge_pa_kernel(tc, x, w_c1, b_c1, w_q, w_k, w_v, bn_gamma, bn_beta, pr
                                  func=ACT.Identity, bias=col(shift, ob), scale=col(gain, ob))
             ns[ob] = n
 
-        def negative_part(ob):
+        def minus_part(ob, on_scalar=False):
             neg = main.tile([P, NPIX], F32, name="neg", tag=("t1", "t2")[ob % 2], bufs=1)
-            nc.vector.tensor_scalar(out=neg[:], in0=ns[ob][:], scalar1=0.0, scalar2=a_col[:, 0:1],
-                                    op0=ALU.min, op1=ALU.mult)
+            if on_scalar:
+                nc.scalar.activation(out=neg[:], in_=ns[ob][:], func=ACT.Relu, scale=-1.0)
+            else:
+                nc.vector.tensor_scalar(out=neg[:], in0=ns[ob][:], scalar1=-1.0, scalar2=0.0, op0=ALU.mult, op1=ALU.max)
             negs[ob] = neg
 
         def prelu_and_store(ob):
             res = mid.tile([P, NPIX], F32, name="res", tag=("ll", "y_mid", "y_left", "y_right")[ob], align_bytes=64)
-            nc.vector.scalar_tensor_tensor(out=res[:], in0=ns[ob][:], scalar=0.0, in1=negs[ob][:],
-                                           op0=ALU.max, op1=ALU.add)
+            nc.vector.scalar_tensor_tensor(out=res[:], in0=negs[ob][:], scalar=one_minus_a[:, 0:1], in1=ns[ob][:],
+                                           op0=ALU.mult, op1=ALU.add)
             nc.sync.dma_start(out=out_v[:, ob], in_=res[:].rearrange("p (b f) -> p b f", b=NB))
 
         B6 = STEPS - 2
@@ -641,46 +627,36 @@ def tile_merge_pa_kernel(tc, x, w_c1, b_c1, w_q, w_k, w_v, bn_gamma, bn_beta, pr
         divide_block(B6, 0)
         divide_block(B7, 0)
         last_squares(0)
-        divide_block(B6, 1)
         last_sum(0)
+        divide_block(B6, 1)
         divide_block(B7, 1)
-        last_squares(1)
-        divide_block(B6, 2)
-        last_sum(1)
         totals(0)
-        divide_block(B7, 2)
-        last_squares(2)
-        mean_squared(0)
-        minus_mean(0)
-        var_plus_eps(0)
-        std(0)
-        minus_mean_gamma(0)
-        last_sum(2)
-        gain_of(0)
-        shift_of(0)
-        shift_of(1)
+        statistics(0)
+        last_squares(1)
+        last_sum(1)
         normalise(0)
+        divide_block(B6, 2)
+        divide_block(B7, 2)
+        totals(1)
+        statistics(1)
+        last_squares(2)
+        last_sum(2)
+        normalise(1)
+        minus_part(0)
         divide_block(B6, 3)
         divide_block(B7, 3)
+        totals(2)
+        statistics(2)
         last_squares(3)
-        normalise(1)
         last_sum(3)
-        negative_part(0)
-        totals(1)
-        mean_squared(1)
-        minus_mean(1)
-        var_plus_eps(1)
-        std(1)
-        minus_mean_gamma(1)
-        gain_of(1)
-        shift_of(2)
-        shift_of(3)
-        normalise(2)
-        normalise(3)
         prelu_and_store(0)
-        negative_part(1)
-        negative_part(2)
+        normalise(2)
+        minus_part(1)
+        totals(3)
+        statistics(3)
         prelu_and_store(1)
-        negative_part(3)
+        normalise(3)
+        minus_part(3, True)
+        minus_part(2)
         prelu_and_store(2)
         prelu_and_store(3)

@@ -123,9 +123,9 @@ def tile_merge_pa_kernel(tc, x, w_c1, b_c1, w_q, w_k, w_v, bn_gamma, bn_beta, pr
         rights = y_right[:].rearrange("p (g x) t -> p g (x t)", x=16)
         nc.gpsimd.memset(lefts[:, :, 0:8], 0.0)
         nc.gpsimd.memset(rights[:, :, 56:64], 0.0)
-        nc.gpsimd.dma_start(out=gam_bf[:], in_=bn_gamma.rearrange("(p t) -> p t", t=4))
-        nc.gpsimd.dma_start(out=bet_bf[:], in_=bn_beta.rearrange("(p t) -> p t", t=4))
-        nc.gpsimd.dma_start(out=a_bf[:], in_=prelu_a.partition_broadcast(P))
+        nc.sync.dma_start(out=gam_bf[:], in_=bn_gamma.rearrange("(p t) -> p t", t=4))
+        nc.sync.dma_start(out=bet_bf[:], in_=bn_beta.rearrange("(p t) -> p t", t=4))
+        nc.sync.dma_start(out=a_bf[:], in_=prelu_a.partition_broadcast(P))
 
         zs = {}
         evs = {}

@@ -277,7 +277,7 @@ def tile_merge_pa_kernel(tc, x, w_c1, b_c1, w_q, w_k, w_v, bn_gamma, bn_beta, pr
             if s == 0:
                 pe_list.extend([("C", 1, t) for t in range(4)] + [("w", W_V, 0), ("w", W_V, 1)] + on_pe(2))
             if s == 1:
-                pe_list.extend([("c", r, 0) for r in range(4, 8)])
+                pe_list.extend([("C", 2, t) for t in range(4)])
             vb = v_banks(a) if ok(a) else []
             den_sums = [("F", a, i) for i in range(36)] if ok(a) else []
             num_sums = [("G", a, i) for i in range(36)] if ok(a) and a < STEPS - 2 else []
@@ -369,10 +369,12 @@ def tile_merge_pa_kernel(tc, x, w_c1, b_c1, w_q, w_k, w_v, bn_gamma, bn_beta, pr
         def add_bias_on_scalar(pc):
             c0 = ROW * PIECES[pc][0]
             n = ROW * PIECES[pc][1]
+            by_slot = main.tile([P, 4, n], BF16, name="by_slot", tag="by_slot", bufs=1)
             for t in range(4):
                 pump_to(("C", pc, t))
-                nc.scalar.activation(out=y_mid[:, c0:c0 + n, t], in_=banks[("C", pc, t)][:], func=ACT.Identity,
+                nc.scalar.activation(out=by_slot[:, t, :], in_=banks[("C", pc, t)][:], func=ACT.Identity,
                                      bias=bias_bf[:, t:t + 1], scale=1.0)
+            return lambda: nc.scalar.copy(out=y_mid[:, c0:c0 + n, :], in_=by_slot[:].rearrange("p t n -> p n t"))
 
         def shift_copies(pc, on_vector):
             g0 = NB * PIECES[pc][0]
@@ -511,12 +513,10 @@ def tile_merge_pa_kernel(tc, x, w_c1, b_c1, w_q, w_k, w_v, bn_gamma, bn_beta, pr
             if s == 2:
                 quant_y(2)
             if s == 0:
-                shift_by_max(s, (lambda: (quant_ll(1), q_copy(1), add_bias_on_scalar(1), shift_copies(1, False)),
+                shift_by_max(s, (lambda: (quant_ll(1), q_copy(1), add_bias_on_scalar(1)(), shift_copies(1, False)),
                                  lambda: haar_on_vector(2, (0, 1)), lambda: (haar_on_vector(2, (2,)), quant_y(1))), 0, True)
             elif s == 1:
                 shift_by_max(s, (lambda: quant_ll(2), lambda: quant_w(W_V, g_v), nothing), 0, True)
-                for r in range(4, 8):
-                    add_bias(r)
                 scores(s + 1, 0, AHEAD)
             else:
                 shift_by_max(s, (early_scores(s + 1, 0), early_scores(s + 1, 1), early_scores(s + 1, 2)),
@@ -525,12 +525,15 @@ def tile_merge_pa_kernel(tc, x, w_c1, b_c1, w_q, w_k, w_v, bn_gamma, bn_beta, pr
                 g_v = weight_copies(W_V)
                 haar_from_pe(2)
                 scores(1, 0, AHEAD)
-            if ok(s - 1):
-                exps(s - 1, 1)
-            if ok(s - 1):
-                exps(s - 1, 2)
             if s == 1:
+                weave = add_bias_on_scalar(2)
+                exps(0, 1)
+                weave()
+                exps(0, 2)
                 shift_copies(2, False)
+            elif ok(s - 1):
+                exps(s - 1, 1)
+                exps(s - 1, 2)
             if ok(s - 2):
                 one_over_den(s - 2)
             if s == 3:

@@ -20,6 +20,7 @@ BN_EPS = 1e-5
 BANK_DT = BF16
 AHEAD = 3
 SHARE_FROM = 1
+WARM_UP = 8
 LATE = 2
 LAST_ON_VECTOR = 3
 PIECES = ((0, 4), (4, 4), (8, 8))
@@ -88,6 +89,8 @@ def tile_merge_pa_kernel(tc, x, w_c1, b_c1, w_q, w_k, w_v, bn_gamma, bn_beta, pr
             wst = keep.tile([P, 512], U8, name="w_scales%d" % i, align_bytes=64)
             w_codes.append(wct)
             w_scales.append(wst)
+        nc.vector.memset(w_codes[W_KN][:], 0)
+        nc.vector.memset(w_scales[W_KN][:].bitcast(I32), 0)
         ll_codes = keep.tile([P, NPIX], I32, name="ll_codes", align_bytes=64)
         ll_scales = keep.tile([P, NPIX], U8, name="ll_scales", align_bytes=64)
         y_codes = []
@@ -177,6 +180,10 @@ def tile_merge_pa_kernel(tc, x, w_c1, b_c1, w_q, w_k, w_v, bn_gamma, bn_beta, pr
                 conv(k_ps[:], s, AROUND[j], W_K, True, False)
                 conv(k_ps[:], s, CENTRE, W_KN, False, True)
                 banks[tok] = k_ps
+            elif kind == "d":
+                idle = psm.tile([P, 512], F32, name="idle", tag="num", bufs=1)
+                nc.tensor.matmul_mx(out=idle[:], lhsT=w_codes[W_KN][:, 0:P].bitcast(FP8X4), lhsT_scale=w_scales[W_KN][:, 0:P],
+                                    rhs=w_codes[W_KN][:].bitcast(FP8X4), rhs_scale=w_scales[W_KN][:], start=True, stop=True)
             elif kind in ("v", "u"):
                 v_ps = psm.tile([P, 512], F32, name="v_ps", tag="v_ps", bufs=3)
                 window(v_ps[:], s, j, W_V)
@@ -265,7 +272,7 @@ def tile_merge_pa_kernel(tc, x, w_c1, b_c1, w_q, w_k, w_v, bn_gamma, bn_beta, pr
         def on_pe(pc):
             return [("h", pc, b) for b in range(NB) if (pc, b) not in HAAR_ON_VECTOR]
 
-        pe_list = [("w", W_C1, 0), ("w", W_C1, 1)] + on_pe(0) + [("w", W_Q, 0), ("w", W_Q, 1), ("c", 0, 0), ("c", 1, 0),
+        pe_list = [("d", 0, i) for i in range(WARM_UP)] + [("w", W_C1, 0), ("w", W_C1, 1)] + on_pe(0) + [("w", W_Q, 0), ("w", W_Q, 1), ("c", 0, 0), ("c", 1, 0),
                                                                  ("w", W_K, 0), ("w", W_K, 1)] + on_pe(1)
         pe_list += [("q", 0, 0)] + [("k", 0, j) for j in range(AHEAD)]
         for s in range(STEPS + 2):

@@ -20,7 +20,7 @@ BN_EPS = 1e-5
 BANK_DT = BF16
 AHEAD = 3
 SHARE_FROM = 1
-WARM_UP = 8
+WARM_UP = 4
 LATE = 2
 LAST_ON_VECTOR = 3
 PIECES = ((0, 4), (4, 4), (8, 8))

@@ -74,6 +74,9 @@ def tile_merge_pa_kernel(tc, x, w_c1, b_c1, w_q, w_k, w_v, bn_gamma, bn_beta, pr
         make_identity(nc, ident[:])
         ident_bf = keep.tile([P, P], BF16, name="ident_bf")
         make_identity(nc, ident_bf[:])
+        to_ybx = keep.tile([P, P], F32, name="to_ybx")
+        nc.gpsimd.tensor_copy(out=to_ybx[:].rearrange("p (y b x) -> p y b x", b=NB, x=16),
+                              in_=ident[:].rearrange("p (y x b) -> p y b x", b=NB, x=16))
 
         gam_bf = keep.tile([P, 4], BF16, name="gam_bf")
         bet_bf = keep.tile([P, 4], BF16, name="bet_bf")
@@ -98,9 +101,12 @@ def tile_merge_pa_kernel(tc, x, w_c1, b_c1, w_q, w_k, w_v, bn_gamma, bn_beta, pr
         for d in range(3):
             yct = keep.tile([P, NPIX + 2 * ROW], I32, name="y_codes%d" % d, align_bytes=64)
             yst = keep.tile([P, NPIX + 2 * ROW], U8, name="y_scales%d" % d, align_bytes=64)
-            for c0 in (0, ROW + NPIX):
-                nc.vector.memset(yct[:, c0:c0 + ROW], 0)
-                nc.vector.memset(yst[:, c0:c0 + ROW].bitcast(I32), 0)
+            if d == 1:
+                for c0 in (0, ROW + NPIX):
+                    nc.vector.memset(yct[:, c0:c0 + ROW], 0)
+            else:
+                nc.vector.memset(yct[:], 0)
+            nc.vector.memset(yst[:].bitcast(I32), 0)
             y_codes.append(yct)
             y_scales.append(yst)
 
@@ -113,19 +119,12 @@ def tile_merge_pa_kernel(tc, x, w_c1, b_c1, w_q, w_k, w_v, bn_gamma, bn_beta, pr
         neg_pivot = keep.tile([P, 4], F32, name="neg_pivot")
         one_minus_a = keep.tile([P, 1], F32, name="one_minus_a")
         gam_f = keep.tile([P, 4], F32, name="gam_f")
-        bias_full = keep.tile([P, P, 4], BF16, name="bias_full")
+        bias_full = keep.tile([P, ROW, 4], BF16, name="bias_full")
 
         ll = mid.tile([P, NPIX, 4], BF16, name="ll", align_bytes=64)
         y_mid = mid.tile([P, NPIX, 4], BF16, name="y_mid", align_bytes=64)
-        y_left = mid.tile([P, NPIX, 4], BF16, name="y_left", align_bytes=64)
-        y_right = mid.tile([P, NPIX, 4], BF16, name="y_right", align_bytes=64)
         ll_by_image = ll[:].rearrange("p (y b x) j -> p b y x j", b=NB, x=16)
         ll_flat = ll[:].rearrange("p c j -> p (c j)")
-        lefts = y_left[:].rearrange("p (g x) t -> p g (x t)", x=16)
-        mids = y_mid[:].rearrange("p (g x) t -> p g (x t)", x=16)
-        rights = y_right[:].rearrange("p (g x) t -> p g (x t)", x=16)
-        nc.gpsimd.memset(lefts[:, :, 0:8], 0.0)
-        nc.gpsimd.memset(rights[:, :, 56:64], 0.0)
         nc.sync.dma_start(out=gam_bf[:], in_=bn_gamma.rearrange("(p t) -> p t", t=4))
         nc.sync.dma_start(out=bet_bf[:], in_=bn_beta.rearrange("(p t) -> p t", t=4))
         nc.sync.dma_start(out=a_bf[:], in_=prelu_a.partition_broadcast(P))
@@ -166,7 +165,7 @@ def tile_merge_pa_kernel(tc, x, w_c1, b_c1, w_q, w_k, w_v, bn_gamma, bn_beta, pr
         def add_up(dst, src, i):
             ob = i // 9
             j = i % 9
-            nc.tensor.matmul(out=dst[:, ob, :], lhsT=src[:, j, P * ob:P * (ob + 1)], rhs=ident[:],
+            nc.tensor.matmul(out=dst[:, ob, :], lhsT=src[:, j, P * ob:P * (ob + 1)], rhs=to_ybx[:],
                              is_transpose=True, start=(j == 0), stop=(j == 8))
 
         def emit_pe(tok):
@@ -238,7 +237,7 @@ def tile_merge_pa_kernel(tc, x, w_c1, b_c1, w_q, w_k, w_v, bn_gamma, bn_beta, pr
                     num = psm.tile([P, 4, P], F32, name="num", tag="num", bufs=1)
                     nums[s] = num
                 ob = j // 3
-                nc.tensor.matmul(out=nums[s][:, ob, :], lhsT=ev_sums[0][:, j % 3, P * ob:P * (ob + 1)], rhs=ident[:],
+                nc.tensor.matmul(out=nums[s][:, ob, :], lhsT=ev_sums[0][:, j % 3, P * ob:P * (ob + 1)], rhs=to_ybx[:],
                                  is_transpose=True, start=(j % 3 == 0), stop=(j % 3 == 2))
             else:
                 if j == 0:
@@ -370,8 +369,11 @@ def tile_merge_pa_kernel(tc, x, w_c1, b_c1, w_q, w_k, w_v, bn_gamma, bn_beta, pr
 
         def add_bias(r):
             pump_to(("c", r, 0))
-            nc.vector.tensor_tensor(out=y_mid[:, P * r:P * (r + 1), :], in0=banks[("c", r, 0)][:].rearrange("p t n -> p n t"),
-                                    in1=bias_full[:], op=ALU.add)
+            for yy in range(2):
+                c0 = P * r + ROW * yy
+                nc.vector.tensor_tensor(out=y_mid[:, c0:c0 + ROW, :].rearrange("p (x b) t -> p x b t", b=NB),
+                                        in0=banks[("c", r, 0)][:, :, ROW * yy:ROW * (yy + 1)].rearrange("p t (b x) -> p x b t", b=NB),
+                                        in1=bias_full[:].rearrange("p (x b) t -> p x b t", b=NB), op=ALU.add)
 
         def add_bias_on_scalar(pc):
             c0 = ROW * PIECES[pc][0]
@@ -379,27 +381,29 @@ def tile_merge_pa_kernel(tc, x, w_c1, b_c1, w_q, w_k, w_v, bn_gamma, bn_beta, pr
             by_slot = main.tile([P, 4, n], BF16, name="by_slot", tag="by_slot", bufs=1)
             for t in range(4):
                 pump_to(("C", pc, t))
-                nc.scalar.activation(out=by_slot[:, t, :], in_=banks[("C", pc, t)][:], func=ACT.Identity,
+                nc.scalar.activation(out=by_slot[:, t, :].rearrange("p (y x b) -> p y x b", x=16, b=NB),
+                                     in_=banks[("C", pc, t)][:].rearrange("p (y b x) -> p y x b", x=16, b=NB), func=ACT.Identity,
                                      bias=bias_bf[:, t:t + 1], scale=1.0)
             return lambda: nc.scalar.copy(out=y_mid[:, c0:c0 + n, :], in_=by_slot[:].rearrange("p t n -> p n t"))
-
-        def shift_copies(pc, on_vector):
-            g0 = NB * PIECES[pc][0]
-            g1 = g0 + NB * PIECES[pc][1]
-            if on_vector:
-                nc.vector.tensor_copy(out=lefts[:, g0:g1, 4:64], in_=mids[:, g0:g1, 0:60])
-                nc.vector.tensor_copy(out=rights[:, g0:g1, 0:60], in_=mids[:, g0:g1, 4:64])
-            else:
-                nc.scalar.copy(out=lefts[:, g0:g1, 4:64], in_=mids[:, g0:g1, 0:60])
-                nc.scalar.copy(out=rights[:, g0:g1, 0:60], in_=mids[:, g0:g1, 4:64])
 
         def quant_y(pc):
             p0 = ROW * PIECES[pc][0]
             n = ROW * PIECES[pc][1]
-            for d, ysrc in ((1, y_mid), (0, y_left), (2, y_right)):
-                nc.vector.quantize_mx(out=y_codes[d][:, ROW + p0:ROW + p0 + n].bitcast(FP8X4),
-                                      scales=y_scales[d][:, ROW + p0:ROW + p0 + n],
-                                      in_=ysrc[:].rearrange("p c j -> p (c j)")[:, 4 * p0:4 * (p0 + n)])
+            nc.vector.quantize_mx(out=y_codes[1][:, ROW + p0:ROW + p0 + n].bitcast(FP8X4),
+                                  scales=y_scales[1][:, ROW + p0:ROW + p0 + n],
+                                  in_=y_mid[:].rearrange("p c j -> p (c j)")[:, 4 * p0:4 * (p0 + n)])
+
+        code_rows = [t[:].rearrange("p (r c) -> p r c", c=ROW) for t in y_codes]
+        scale_rows = [t[:].bitcast(I32).rearrange("p (r c) -> p r c", c=ROW // 4) for t in y_scales]
+
+        def move_y(pc):
+            r0 = 1 + PIECES[pc][0]
+            r1 = r0 + PIECES[pc][1]
+            w = ROW // 4
+            nc.vector.tensor_copy(out=code_rows[0][:, r0:r1, NB:ROW], in_=code_rows[1][:, r0:r1, 0:ROW - NB])
+            nc.vector.tensor_copy(out=code_rows[2][:, r0:r1, 0:ROW - NB], in_=code_rows[1][:, r0:r1, NB:ROW])
+            nc.vector.tensor_copy(out=scale_rows[0][:, r0:r1, 1:w], in_=scale_rows[1][:, r0:r1, 0:w - 1])
+            nc.vector.tensor_copy(out=scale_rows[2][:, r0:r1, 0:w - 1], in_=scale_rows[1][:, r0:r1, 1:w])
 
         def q_copy(s):
             pump_to(("q", s, 0))
@@ -482,18 +486,18 @@ def tile_merge_pa_kernel(tc, x, w_c1, b_c1, w_q, w_k, w_v, bn_gamma, bn_beta, pr
         g_c1 = weight_copies(W_C1)
         haar_on_vector(0, (0, 1))
         quant_w(W_C1, g_c1)
-        nc.vector.tensor_copy(out=bias_full[:], in_=bias_bf[:].unsqueeze(1).to_broadcast([P, P, 4]))
+        nc.vector.tensor_copy(out=bias_full[:], in_=bias_bf[:].unsqueeze(1).to_broadcast([P, ROW, 4]))
         haar_from_pe(0)
         quant_ll(0)
         g_q = weight_copies(W_Q)
         add_bias(0)
         add_bias(1)
         quant_w(W_Q, g_q)
-        shift_copies(0, True)
         g_k = weight_copies(W_K)
         quant_y(0)
         g_kn = main.tile([P, 2048], BF16, name="grouped_neg", tag="grouped", bufs=2, align_bytes=64)
         nc.vector.tensor_scalar(out=g_kn[:], in0=g_k[:], scalar1=-1.0, scalar2=None, op0=ALU.mult)
+        move_y(0)
         quant_w(W_K, g_k)
         quant_w(W_KN, g_kn)
         q_copy(0)
@@ -520,15 +524,18 @@ def tile_merge_pa_kernel(tc, x, w_c1, b_c1, w_q, w_k, w_v, bn_gamma, bn_beta, pr
             if s == 2:
                 quant_y(2)
             if s == 0:
-                shift_by_max(s, (lambda: (quant_ll(1), q_copy(1), add_bias_on_scalar(1)(), shift_copies(1, False)),
+                shift_by_max(s, (lambda: (quant_ll(1), q_copy(1), add_bias_on_scalar(1)()),
                                  lambda: haar_on_vector(2, (0, 1)), lambda: (haar_on_vector(2, (2,)), quant_y(1))), 0, True)
             elif s == 1:
                 shift_by_max(s, (lambda: quant_ll(2), lambda: quant_w(W_V, g_v), nothing), 0, True)
                 scores(s + 1, 0, AHEAD)
+            elif s == 2:
+                shift_by_max(s, (lambda: (move_y(2), scores(s + 1, 0, 1)), early_scores(s + 1, 1), early_scores(s + 1, 2)))
             else:
                 shift_by_max(s, (early_scores(s + 1, 0), early_scores(s + 1, 1), early_scores(s + 1, 2)),
                              LAST_ON_VECTOR if s == STEPS - 1 else 0)
             if s == 0:
+                move_y(1)
                 g_v = weight_copies(W_V)
                 haar_from_pe(2)
                 scores(1, 0, AHEAD)
@@ -537,7 +544,6 @@ def tile_merge_pa_kernel(tc, x, w_c1, b_c1, w_q, w_k, w_v, bn_gamma, bn_beta, pr
                 exps(0, 1)
                 weave()
                 exps(0, 2)
-                shift_copies(2, False)
             elif ok(s - 1):
                 exps(s - 1, 1)
                 exps(s - 1, 2)
@@ -627,7 +633,7 @@ def tile_merge_pa_kernel(tc, x, w_c1, b_c1, w_q, w_k, w_v, bn_gamma, bn_beta, pr
             negs[ob] = neg
 
         def prelu_and_store(ob):
-            res = mid.tile([P, NPIX], F32, name="res", tag=("ll", "y_mid", "y_left", "y_right")[ob], align_bytes=64)
+            res = mid.tile([P, NPIX], F32, name="res", tag=("ll", "y_mid", "res_c", "res_d")[ob], align_bytes=64)
             nc.vector.scalar_tensor_tensor(out=res[:], in0=negs[ob][:], scalar=one_minus_a[:, 0:1], in1=ns[ob][:],
                                            op0=ALU.mult, op1=ALU.add)
             nc.sync.dma_start(out=out_v[:, ob], in_=res[:].rearrange("p (b f) -> p b f", b=NB))

@@ -605,9 +605,10 @@ def tile_merge_pa_kernel(tc, x, w_c1, b_c1, w_q, w_k, w_v, bn_gamma, bn_beta, pr
             nc.vector.tensor_reduce(out=tot[:, :, ob:ob + 1], in_=msums[:, :, ob:ob + 1, :], axis=mybir.AxisListType.X, op=ALU.add)
 
         def statistics(ob):
-            nc.scalar.activation(out=col(dd, ob), in_=tot[:, 0, ob:ob + 1], func=ACT.Square, scale=1.0 / NPIX)
-            nc.scalar.activation(out=col(neg_mean, ob), in_=tot[:, 0, ob:ob + 1], func=ACT.Identity, bias=col(neg_pivot, ob),
-                                 scale=-1.0 / NPIX)
+            nc.vector.scalar_tensor_tensor(out=col(dd, ob), in0=tot[:, 0, ob:ob + 1], scalar=1.0 / (NPIX * NPIX), in1=tot[:, 0, ob:ob + 1],
+                                           op0=ALU.mult, op1=ALU.mult)
+            nc.vector.tensor_scalar(out=col(neg_mean, ob), in0=tot[:, 0, ob:ob + 1], scalar1=-1.0 / NPIX, scalar2=col(neg_pivot, ob),
+                                    op0=ALU.mult, op1=ALU.add)
             nc.scalar.activation(out=col(rstd, ob), in_=tot[:, 1, ob:ob + 1], func=ACT.Abs_reciprocal_sqrt, bias=col(dd, ob),
                                  scale=-1.0 / NPIX)
             nc.scalar.activation(out=col(gain, ob), in_=col(rstd, ob), func=ACT.Copy, scale=col(gam_f, ob))

@@ -254,11 +254,11 @@ def tile_merge_pa_kernel(tc, x, w_c1, b_c1, w_q, w_k, w_v, bn_gamma, bn_beta, pr
                 todo.extend([(("u", 2 * a - 1, d), a, d) for d in range(3)])
             todo.append((("v", 2 * a, 0), a, 3))
             todo.append((("v", 2 * a, 2), a, 4))
+            todo.append((("v", 2 * a, 1), a, 8))
             for d in range(3):
                 todo.append((("v", 2 * a + 1, d), a, 5 + d))
                 if ok(a + 1) and a >= SHARE_FROM:
                     todo.append((("v", 2 * a + 1, d), a + 1, d))
-            todo.append((("v", 2 * a, 1), a, 8))
             return todo
 
         def v_banks(a):
@@ -557,12 +557,12 @@ def tile_merge_pa_kernel(tc, x, w_c1, b_c1, w_q, w_k, w_v, bn_gamma, bn_beta, pr
                 moments(s - 4)
         divide(STEPS - 3)
         exps(STEPS - 1, 0)
-        weigh(STEPS - 2, 0, 3)
+        weigh(STEPS - 2, 0, 4)
         ev_sum = main.tile([P, 3, 512], F32, name="ev_sum", tag="t1", bufs=1)
         ev_sums.append(ev_sum)
         ev6 = evs[STEPS - 2]
         nc.gpsimd.tensor_tensor(out=ev_sum[:], in0=ev6[:, 0:3, :], in1=ev6[:, 3:6, :], op=ALU.add)
-        weigh(STEPS - 2, 3, 9)
+        weigh(STEPS - 2, 4, 9)
         nc.gpsimd.tensor_tensor(out=ev_sum[:], in0=ev_sum[:], in1=ev6[:, 6:9, :], op=ALU.add)
         exps(STEPS - 1, 1)
         exps(STEPS - 1, 2)

@@ -301,12 +301,9 @@ def tile_merge_pa_kernel(tc, x, w_c1, b_c1, w_q, w_k, w_v, bn_gamma, bn_beta, pr
             if ok(s + 1):
                 pe_list.extend([("k", s + 1, j) for j in range(AHEAD)])
             pe_list.extend(den_sums[18:])
-            pe_list.extend(num_sums[:27])
+            pe_list.extend(num_sums)
             if ok(s + 1):
-                pe_list.append(("k", s + 1, AHEAD))
-            pe_list.extend(num_sums[27:])
-            if ok(s + 1):
-                pe_list.append(("k", s + 1, AHEAD + 1))
+                pe_list.extend([("k", s + 1, AHEAD + j) for j in range(LATE)])
         for ob in range(4):
             pe_list.extend([("G", STEPS - 2, 3 * ob + j) for j in range(3)])
             pe_list.extend([("G", STEPS - 1, 9 * ob + j) for j in range(9)])

@@ -506,6 +506,17 @@ def tile_merge_pa_kernel(tc, x, w_c1, b_c1, w_q, w_k, w_v, bn_gamma, bn_beta, pr
         def early_scores(s, j):
             return (lambda: scores(s, j, j + 1)) if ok(s) else nothing
 
+        def half_score(s, h):
+            cols = slice(256 * h, 256 * (h + 1))
+            pump_to(("k", s, 0))
+            if h == 0:
+                z = main.tile([P, 9, 512], F32, name="z", tag="z", bufs=3)
+                zs[s] = z
+            nc.vector.tensor_tensor(out=zs[s][:, 0, cols], in0=q_sbs[s][:, cols], in1=banks[("k", s, 0)][:, cols], op=ALU.mult)
+
+        def early_half(s, h):
+            return (lambda: half_score(s, h)) if ok(s) else nothing
+
         haar_on_vector(1, (2, 3), True)
         scores(0, 0, AHEAD)
         for s in range(STEPS):
@@ -529,7 +540,7 @@ def tile_merge_pa_kernel(tc, x, w_c1, b_c1, w_q, w_k, w_v, bn_gamma, bn_beta, pr
             elif s == 2:
                 shift_by_max(s, (lambda: (move_y(2), scores(s + 1, 0, 1)), early_scores(s + 1, 1), early_scores(s + 1, 2)))
             else:
-                shift_by_max(s, (early_scores(s + 1, 0), early_scores(s + 1, 1), early_scores(s + 1, 2)),
+                shift_by_max(s, (early_half(s + 1, 0), early_half(s + 1, 1), (lambda: scores(s + 1, 1, AHEAD)) if ok(s + 1) else nothing),
                              LAST_ON_VECTOR if s == STEPS - 1 else 0)
             if s == 0:
                 move_y(1)

@@ -416,6 +416,29 @@ def tile_merge_pa_kernel(tc, x, w_c1, b_c1, w_q, w_k, w_v, bn_gamma, bn_beta, pr
                     zs[s] = z
                 nc.vector.tensor_tensor(out=zs[s][:, j, :], in0=q_sbs[s][:], in1=banks[("k", s, j)][:], op=ALU.mult)
 
+        def subtract(s, g, eng):
+            g0, g1 = GROUPS[g]
+            z = zs[s]
+            eng.tensor_tensor(out=z[:, g0:g1, :], in0=z[:, g0:g1, :], in1=ms[s][:].unsqueeze(1).to_broadcast([P, g1 - g0, 512]),
+                              op=ALU.subtract)
+
+        def tree_in_halves(s, between, on_vector=0):
+            z = zs[s]
+            halves = (slice(0, 256), slice(256, 512))
+            t1 = main.tile([P, 4, 512], F32, name="t1", tag="t1", bufs=1)
+            for c in halves:
+                nc.vector.tensor_tensor(out=t1[:, :, c], in0=z[:, 0:4, c], in1=z[:, 4:8, c], op=ALU.max)
+            between()
+            t2 = main.tile([P, 2, 512], F32, name="t2", tag="t2", bufs=1)
+            for c in halves:
+                nc.vector.tensor_tensor(out=t2[:, :, c], in0=t1[:, 0:2, c], in1=t1[:, 2:4, c], op=ALU.max)
+            m = main.tile([P, 512], F32, name="m", tag="m")
+            for c in halves:
+                nc.vector.scalar_tensor_tensor(out=m[:, c], in0=t2[:, 0, c], scalar=0.0, in1=t2[:, 1, c], op0=ALU.max, op1=ALU.max)
+            ms[s] = m
+            for g in range(len(GROUPS)):
+                subtract(s, g, nc.vector if 3 * g < on_vector else nc.gpsimd)
+
         def shift_by_max(s, between, on_vector=0, all_before_m=False):
             z = zs[s]
             t1 = main.tile([P, 4, 512], F32, name="t1", tag="t1", bufs=1)
@@ -431,10 +454,8 @@ def tile_merge_pa_kernel(tc, x, w_c1, b_c1, w_q, w_k, w_v, bn_gamma, bn_beta, pr
             ms[s] = m
             if not all_before_m:
                 between[2]()
-            for g, (g0, g1) in enumerate(GROUPS):
-                eng = nc.vector if 3 * g < on_vector else nc.gpsimd
-                eng.tensor_tensor(out=z[:, g0:g1, :], in0=z[:, g0:g1, :], in1=m[:].unsqueeze(1).to_broadcast([P, g1 - g0, 512]),
-                                  op=ALU.subtract)
+            for g in range(len(GROUPS)):
+                subtract(s, g, nc.vector if 3 * g < on_vector else nc.gpsimd)
 
         def exps(s, g):
             z = zs[s]
@@ -503,19 +524,6 @@ def tile_merge_pa_kernel(tc, x, w_c1, b_c1, w_q, w_k, w_v, bn_gamma, bn_beta, pr
         def nothing():
             return None
 
-        def early_scores(s, j):
-            return (lambda: scores(s, j, j + 1)) if ok(s) else nothing
-
-        def half_score(s, h):
-            cols = slice(256 * h, 256 * (h + 1))
-            pump_to(("k", s, 0))
-            if h == 0:
-                z = main.tile([P, 9, 512], F32, name="z", tag="z", bufs=3)
-                zs[s] = z
-            nc.vector.tensor_tensor(out=zs[s][:, 0, cols], in0=q_sbs[s][:, cols], in1=banks[("k", s, 0)][:, cols], op=ALU.mult)
-
-        def early_half(s, h):
-            return (lambda: half_score(s, h)) if ok(s) else nothing
 
         haar_on_vector(1, (2, 3), True)
         scores(0, 0, AHEAD)
@@ -537,11 +545,10 @@ def tile_merge_pa_kernel(tc, x, w_c1, b_c1, w_q, w_k, w_v, bn_gamma, bn_beta, pr
             elif s == 1:
                 shift_by_max(s, (lambda: quant_ll(2), lambda: quant_w(W_V, g_v), nothing), 0, True)
                 scores(s + 1, 0, AHEAD)
-            elif s == 2:
-                shift_by_max(s, (lambda: (move_y(2), scores(s + 1, 0, 1)), early_scores(s + 1, 1), early_scores(s + 1, 2)))
             else:
-                shift_by_max(s, (early_half(s + 1, 0), early_half(s + 1, 1), (lambda: scores(s + 1, 1, AHEAD)) if ok(s + 1) else nothing),
-                             LAST_ON_VECTOR if s == STEPS - 1 else 0)
+                tree_in_halves(s, (lambda: move_y(2)) if s == 2 else nothing, LAST_ON_VECTOR if s == STEPS - 1 else 0)
+                if ok(s + 1):
+                    scores(s + 1, 0, AHEAD)
             if s == 0:
                 move_y(1)
                 g_v = weight_copies(W_V)

@@ -358,6 +358,13 @@ def tile_merge_pa_kernel(tc, x, w_c1, b_c1, w_q, w_k, w_v, bn_gamma, bn_beta, pr
                 eng.tensor_tensor(out=s2[:], in0=pairs[:, :, 0], in1=pairs[:, :, 1], op=ALU.add)
                 halve(pc, b, s2[:])
 
+        def haar_by_reduce(pc, b):
+            nr = PIECES[pc][1]
+            taps = x_piece(pc, b).rearrange("p j (i a x e) -> p j i x a e", a=2, x=16, e=2)
+            s2 = main.tile([P, ROW * nr], F32, name="s2_red", tag="s2", bufs=3)
+            nc.vector.tensor_reduce(out=s2[:].rearrange("p (j i x) -> p j i x", j=4, x=16), in_=taps, axis=mybir.AxisListType.XY, op=ALU.add)
+            return s2
+
         def quant_ll(pc):
             c0 = ROW * PIECES[pc][0]
             n = ROW * PIECES[pc][1]
@@ -529,10 +536,14 @@ def tile_merge_pa_kernel(tc, x, w_c1, b_c1, w_q, w_k, w_v, bn_gamma, bn_beta, pr
         scores(0, 0, AHEAD)
         for s in range(STEPS):
             scores(s, AHEAD, 8)
+            if s == 1:
+                late_sums = haar_by_reduce(2, 2)
             if ok(s - 1):
                 exps(s - 1, 0)
             if s > 0 and ok(s + 1):
                 q_copy(s + 1)
+            if s == 1:
+                halve(2, 2, late_sums[:])
             if ok(s - 3):
                 divide(s - 3)
             if ok(s - 2):
@@ -541,7 +552,7 @@ def tile_merge_pa_kernel(tc, x, w_c1, b_c1, w_q, w_k, w_v, bn_gamma, bn_beta, pr
                 quant_y(2)
             if s == 0:
                 shift_by_max(s, (lambda: (quant_ll(1), q_copy(1), add_bias_on_scalar(1)()),
-                                 lambda: haar_on_vector(2, (0, 1)), lambda: (haar_on_vector(2, (2,)), quant_y(1))), 0, True)
+                                 lambda: haar_on_vector(2, (0, 1)), lambda: quant_y(1)), 0, True)
             elif s == 1:
                 shift_by_max(s, (lambda: quant_ll(2), lambda: quant_w(W_V, g_v), nothing), 0, True)
                 scores(s + 1, 0, AHEAD)

@@ -51,8 +51,11 @@ def tile_merge_pa_kernel(tc, x, w_c1, b_c1, w_q, w_k, w_v, bn_gamma, bn_beta, pr
         def x_piece(pc, b):
             return x_c[:, b] if pc == 2 else x_ab[:, pc, b]
 
-        def load_w(i):
-            nc.sync.dma_start(out=w_all[:, i], in_=weights[i].rearrange("(c r) k -> c r k", r=4))
+        def load_w(i, parts=1):
+            n = 4 // parts
+            for h in range(parts):
+                nc.sync.dma_start(out=w_all[:, i, n * h:n * (h + 1)],
+                                  in_=weights[i].rearrange("(c r) k -> c r k", r=4)[:, n * h:n * (h + 1)])
 
         def load_x(pc):
             row0, nr = PIECES[pc]
@@ -65,7 +68,7 @@ def tile_merge_pa_kernel(tc, x, w_c1, b_c1, w_q, w_k, w_v, bn_gamma, bn_beta, pr
         load_w(W_C1)
         load_x(0)
         load_w(W_Q)
-        load_w(W_K)
+        load_w(W_K, 2)
         load_x(1)
         load_w(W_V)
         load_x(2)
@@ -329,6 +332,10 @@ def tile_merge_pa_kernel(tc, x, w_c1, b_c1, w_q, w_k, w_v, bn_gamma, bn_beta, pr
         def quant_w(i, grouped):
             nc.vector.quantize_mx(out=w_codes[i][:].bitcast(FP8X4), scales=w_scales[i][:], in_=grouped[:])
 
+        def quant_w_half(i, grouped, h):
+            nc.vector.quantize_mx(out=w_codes[i][:, 256 * h:256 * (h + 1)].bitcast(FP8X4), scales=w_scales[i][:, 256 * h:256 * (h + 1)],
+                                  in_=grouped[:, 1024 * h:1024 * (h + 1)])
+
         def halve(pc, b, sums):
             row0, nr = PIECES[pc]
             nc.scalar.activation(out=ll_by_image[:, b, row0:row0 + nr],
@@ -521,10 +528,17 @@ def tile_merge_pa_kernel(tc, x, w_c1, b_c1, w_q, w_k, w_v, bn_gamma, bn_beta, pr
         g_k = weight_copies(W_K)
         quant_y(0)
         g_kn = main.tile([P, 2048], BF16, name="grouped_neg", tag="grouped", bufs=2, align_bytes=64)
-        nc.vector.tensor_scalar(out=g_kn[:], in0=g_k[:], scalar1=-1.0, scalar2=None, op0=ALU.mult)
+        def negate_half(h):
+            nc.vector.tensor_scalar(out=g_kn[:, 1024 * h:1024 * (h + 1)], in0=g_k[:, 1024 * h:1024 * (h + 1)], scalar1=-1.0, scalar2=None,
+                                    op0=ALU.mult)
+
+        negate_half(0)
+        quant_w_half(W_K, g_k, 0)
+        quant_w_half(W_KN, g_kn, 0)
         move_y(0)
-        quant_w(W_K, g_k)
-        quant_w(W_KN, g_kn)
+        negate_half(1)
+        quant_w_half(W_K, g_k, 1)
+        quant_w_half(W_KN, g_kn, 1)
         q_copy(0)
         haar_from_pe(1)
 

@@ -21,6 +21,8 @@ BANK_DT = BF16
 AHEAD = 3
 SHARE_FROM = 1
 WARM_UP = 4
+EARLY_FROM = 1
+FIRST_LENT = 2
 LATE = 2
 LAST_ON_VECTOR = 3
 PIECES = ((0, 4), (4, 4), (8, 8))
@@ -178,7 +180,10 @@ def tile_merge_pa_kernel(tc, x, w_c1, b_c1, w_q, w_k, w_v, bn_gamma, bn_beta, pr
                 conv(q_ps[:], s, 4, W_Q)
                 banks[tok] = q_ps
             elif kind == "k":
-                k_ps = psm.tile([P, 512], F32, name="k_ps", tag="k_ps", bufs=3)
+                if j == AHEAD and s >= FIRST_LENT:
+                    k_ps = psm.tile([P, 512], F32, name="k_lent", tag="den", bufs=1)
+                else:
+                    k_ps = psm.tile([P, 512], F32, name="k_ps", tag="k_ps", bufs=3)
                 conv(k_ps[:], s, AROUND[j], W_K, True, False)
                 conv(k_ps[:], s, CENTRE, W_KN, False, True)
                 banks[tok] = k_ps
@@ -187,7 +192,10 @@ def tile_merge_pa_kernel(tc, x, w_c1, b_c1, w_q, w_k, w_v, bn_gamma, bn_beta, pr
                 nc.tensor.matmul_mx(out=idle[:], lhsT=w_codes[W_KN][:, 0:P].bitcast(FP8X4), lhsT_scale=w_scales[W_KN][:, 0:P],
                                     rhs=w_codes[W_KN][:].bitcast(FP8X4), rhs_scale=w_scales[W_KN][:], start=True, stop=True)
             elif kind in ("v", "u"):
-                v_ps = psm.tile([P, 512], F32, name="v_ps", tag="v_ps", bufs=3)
+                if tok in lent_to_v:
+                    v_ps = psm.tile([P, 512], F32, name="v_lent", tag="num", bufs=1)
+                else:
+                    v_ps = psm.tile([P, 512], F32, name="v_ps", tag="v_ps", bufs=3)
                 window(v_ps[:], s, j, W_V)
                 banks[tok] = v_ps
             elif kind == "c":
@@ -271,6 +279,8 @@ def tile_merge_pa_kernel(tc, x, w_c1, b_c1, w_q, w_k, w_v, bn_gamma, bn_beta, pr
                     toks.append(tok)
             return toks
 
+        lent_to_v = [v_banks(a)[3] for a in range(STEPS)]
+
         def on_pe(pc):
             return [("h", pc, b) for b in range(NB) if (pc, b) not in HAAR_ON_VECTOR]
 
@@ -287,7 +297,8 @@ def tile_merge_pa_kernel(tc, x, w_c1, b_c1, w_q, w_k, w_v, bn_gamma, bn_beta, pr
                 pe_list.extend([("C", 1, t) for t in range(4)] + [("w", W_V, 0), ("w", W_V, 1)] + on_pe(2))
             if s == 1:
                 pe_list.extend([("C", 2, t) for t in range(4)])
-            vb = v_banks(a) if ok(a) else []
+            vb = v_banks(a)[3 if a >= EARLY_FROM else 0:] if ok(a) else []
+            early = v_banks(a + 1)[:3] if ok(a + 1) and a + 1 >= EARLY_FROM else []
             den_sums = [("F", a, i) for i in range(36)] if ok(a) else []
             num_sums = [("G", a, i) for i in range(36)] if ok(a) and a < STEPS - 2 else []
             if a == STEPS - 2:
@@ -296,15 +307,15 @@ def tile_merge_pa_kernel(tc, x, w_c1, b_c1, w_q, w_k, w_v, bn_gamma, bn_beta, pr
             if a == STEPS - 1:
                 pe_list.extend(vb)
                 vb = []
-            pe_list.extend(vb[:3])
-            pe_list.extend(den_sums[:9])
-            pe_list.extend(vb[3:5])
-            pe_list.extend(den_sums[9:18])
-            pe_list.extend(vb[5:])
+            if ok(a) and a < EARLY_FROM:
+                pe_list.extend(vb[:3] + den_sums[:9] + vb[3:5] + den_sums[9:18] + vb[5:])
+            else:
+                pe_list.extend(den_sums[:18] + vb)
             if ok(s + 1):
                 pe_list.extend([("k", s + 1, j) for j in range(AHEAD)])
             pe_list.extend(den_sums[18:])
             pe_list.extend(num_sums)
+            pe_list.extend(early)
             if ok(s + 1):
                 pe_list.extend([("k", s + 1, AHEAD + j) for j in range(LATE)])
         for ob in range(4):

@@ -24,6 +24,7 @@ WARM_UP = 4
 EARLY_FROM = 1
 FIRST_LENT = 2
 LATE = 2
+LAST_BANKS = (("num", 1), ("k_ps", 3), ("k_ps", 3), ("v_ps", 3), ("v_ps", 3), ("v_ps", 3), ("den", 1), ("k_ps", 3))
 LAST_ON_VECTOR = 3
 PIECES = ((0, 4), (4, 4), (8, 8))
 HAAR_ON_VECTOR = ((0, 0), (0, 1), (1, 2), (1, 3), (2, 0), (2, 1), (2, 2))
@@ -173,6 +174,11 @@ def tile_merge_pa_kernel(tc, x, w_c1, b_c1, w_q, w_k, w_v, bn_gamma, bn_beta, pr
             nc.tensor.matmul(out=dst[:, ob, :], lhsT=src[:, j, P * ob:P * (ob + 1)], rhs=to_ybx[:],
                              is_transpose=True, start=(j == 0), stop=(j == 8))
 
+        def last_bank(s, ob):
+            tag, bufs = LAST_BANKS[2 * ob + s - (STEPS - 2)]
+            bank = psm.tile([P, P], F32, name="num_end", tag=tag, bufs=bufs)
+            nums[(s, ob)] = bank
+
         def emit_pe(tok):
             kind, s, j = tok
             if kind == "q":
@@ -244,18 +250,21 @@ def tile_merge_pa_kernel(tc, x, w_c1, b_c1, w_q, w_k, w_v, bn_gamma, bn_beta, pr
                     dens[s] = den
                 add_up(dens[s], zs[s], j)
             elif kind == "G" and s == STEPS - 2:
-                if j == 0:
-                    num = psm.tile([P, 4, P], F32, name="num", tag="num", bufs=1)
-                    nums[s] = num
-                ob = j // 3
-                nc.tensor.matmul(out=nums[s][:, ob, :], lhsT=ev_sums[0][:, j % 3, P * ob:P * (ob + 1)], rhs=to_ybx[:],
-                                 is_transpose=True, start=(j % 3 == 0), stop=(j % 3 == 2))
+                ob = j // 6
+                if j % 6 == 0:
+                    last_bank(s, ob)
+                term = ev_sums[0][:, j % 6, :] if j % 6 < 3 else evs[s][:, 3 + j % 6, :]
+                nc.tensor.matmul(out=nums[(s, ob)][:], lhsT=term[:, P * ob:P * (ob + 1)], rhs=to_ybx[:],
+                                 is_transpose=True, start=(j % 6 == 0), stop=(j % 6 == 5))
+            elif kind == "G" and s == STEPS - 1:
+                ob = j // 9
+                if j % 9 == 0:
+                    last_bank(s, ob)
+                nc.tensor.matmul(out=nums[(s, ob)][:], lhsT=evs[s][:, j % 9, P * ob:P * (ob + 1)], rhs=to_ybx[:],
+                                 is_transpose=True, start=(j % 9 == 0), stop=(j % 9 == 8))
             else:
                 if j == 0:
-                    if s == STEPS - 1:
-                        num = psm.tile([P, 4, P], F32, name="num_last", tag="k_ps", bufs=3)
-                    else:
-                        num = psm.tile([P, 4, P], F32, name="num", tag="num", bufs=1)
+                    num = psm.tile([P, 4, P], F32, name="num", tag="num", bufs=1)
                     nums[s] = num
                 add_up(nums[s], evs[s], j)
 
@@ -319,7 +328,7 @@ def tile_merge_pa_kernel(tc, x, w_c1, b_c1, w_q, w_k, w_v, bn_gamma, bn_beta, pr
             if ok(s + 1):
                 pe_list.extend([("k", s + 1, AHEAD + j) for j in range(LATE)])
         for ob in range(4):
-            pe_list.extend([("G", STEPS - 2, 3 * ob + j) for j in range(3)])
+            pe_list.extend([("G", STEPS - 2, 6 * ob + j) for j in range(6)])
             pe_list.extend([("G", STEPS - 1, 9 * ob + j) for j in range(9)])
 
         done = set()
@@ -462,7 +471,10 @@ def tile_merge_pa_kernel(tc, x, w_c1, b_c1, w_q, w_k, w_v, bn_gamma, bn_beta, pr
                 nc.vector.scalar_tensor_tensor(out=m[:, c], in0=t2[:, 0, c], scalar=0.0, in1=t2[:, 1, c], op0=ALU.max, op1=ALU.max)
             ms[s] = m
             for g in range(len(GROUPS)):
-                subtract(s, g, nc.vector if 3 * g < on_vector else nc.gpsimd)
+                if 3 * g < on_vector:
+                    subtract(s, g, nc.vector)
+                elif on_vector == 0:
+                    subtract(s, g, nc.gpsimd)
 
         def shift_by_max(s, between, on_vector=0, all_before_m=False):
             z = zs[s]
@@ -517,14 +529,15 @@ def tile_merge_pa_kernel(tc, x, w_c1, b_c1, w_q, w_k, w_v, bn_gamma, bn_beta, pr
             cols = slice(P * s, P * (s + 1))
             nc.vector.tensor_tensor(out=att[:, :, cols], in0=nums[s][:], in1=rds[s][:], op=ALU.mult)
 
-        def moments(s):
+        def moments(s, first=0, end=8):
             cols = slice(P * s, P * (s + 2))
-            for ob in range(4):
-                for kind, func in enumerate((ACT.Identity, ACT.Square)):
-                    junk = main.tile([P, 2 * P], F32, name="junk", tag="junk")
-                    nc.scalar.activation(out=junk[:], in_=att[:, ob, cols], func=func,
-                                         bias=neg_pivot[:, ob:ob + 1], scale=1.0,
-                                         accum_out=msums[:, kind, ob, s // 2:s // 2 + 1])
+            for i in range(first, end):
+                ob = i // 2
+                kind = i % 2
+                junk = main.tile([P, 2 * P], F32, name="junk", tag="junk")
+                nc.scalar.activation(out=junk[:], in_=att[:, ob, cols], func=(ACT.Identity, ACT.Square)[kind],
+                                     bias=neg_pivot[:, ob:ob + 1], scale=1.0,
+                                     accum_out=msums[:, kind, ob, s // 2:s // 2 + 1])
 
         g_c1 = weight_copies(W_C1)
         haar_on_vector(0, (0, 1))
@@ -606,23 +619,30 @@ def tile_merge_pa_kernel(tc, x, w_c1, b_c1, w_q, w_k, w_v, bn_gamma, bn_beta, pr
                 nc.scalar.copy(out=gam_f[:], in_=gam_bf[:])
             if ok(s - 3) and (s - 3) % 2 == 1:
                 moments(s - 4)
+        neg_m = main.tile([P, 512], F32, name="neg_m", tag="m")
+        nc.scalar.activation(out=neg_m[:], in_=ms[STEPS - 1][:], func=ACT.Copy, scale=-1.0)
+        z_last = zs[STEPS - 1]
+        for g0, g1 in GROUPS[LAST_ON_VECTOR // 3:]:
+            nc.gpsimd.tensor_tensor(out=z_last[:, g0:g1, :], in0=z_last[:, g0:g1, :],
+                                    in1=neg_m[:].unsqueeze(1).to_broadcast([P, g1 - g0, 512]), op=ALU.add)
         divide(STEPS - 3)
         exps(STEPS - 1, 0)
+        moments(STEPS - 4, 0, 3)
         weigh(STEPS - 2, 0, 4)
         ev_sum = main.tile([P, 3, 512], F32, name="ev_sum", tag="t1", bufs=1)
         ev_sums.append(ev_sum)
         ev6 = evs[STEPS - 2]
         nc.gpsimd.tensor_tensor(out=ev_sum[:], in0=ev6[:, 0:3, :], in1=ev6[:, 3:6, :], op=ALU.add)
         weigh(STEPS - 2, 4, 9)
-        nc.gpsimd.tensor_tensor(out=ev_sum[:], in0=ev_sum[:], in1=ev6[:, 6:9, :], op=ALU.add)
         exps(STEPS - 1, 1)
+        moments(STEPS - 4, 3, 6)
         exps(STEPS - 1, 2)
-        moments(STEPS - 4)
-        weigh(STEPS - 1, 0, 9)
         log_den(STEPS - 2)
         exp_minus_log(STEPS - 2)
+        weigh(STEPS - 1, 0, 9)
         log_den(STEPS - 1)
         exp_minus_log(STEPS - 1)
+        moments(STEPS - 4, 6, 8)
 
         last = slice(P * (STEPS - 2), NPIX)
         tot = keep.tile([P, 2, 4], F32, name="tot")
@@ -639,8 +659,8 @@ def tile_merge_pa_kernel(tc, x, w_c1, b_c1, w_q, w_k, w_v, bn_gamma, bn_beta, pr
             return t[:, ob:ob + 1]
 
         def divide_block(s, ob):
-            pump_to(("G", s, 3 * ob + 2 if s == STEPS - 2 else 9 * ob + 8))
-            nc.vector.tensor_tensor(out=att[:, ob, P * s:P * (s + 1)], in0=nums[s][:, ob, :], in1=rds[s][:, ob, :], op=ALU.mult)
+            pump_to(("G", s, 6 * ob + 5 if s == STEPS - 2 else 9 * ob + 8))
+            nc.vector.tensor_tensor(out=att[:, ob, P * s:P * (s + 1)], in0=nums[(s, ob)][:], in1=rds[s][:, ob, :], op=ALU.mult)
 
         def last_sum(ob):
             junk_v = main.tile([P, 2 * P], F32, name="junk_v", tag="junk_v")

@@ -257,11 +257,11 @@ def tile_merge_pa_kernel(tc, x, w_c1, b_c1, w_q, w_k, w_v, bn_gamma, bn_beta, pr
                 nc.tensor.matmul(out=nums[(s, ob)][:], lhsT=term[:, P * ob:P * (ob + 1)], rhs=to_ybx[:],
                                  is_transpose=True, start=(j % 6 == 0), stop=(j % 6 == 5))
             elif kind == "G" and s == STEPS - 1:
-                ob = j // 9
-                if j % 9 == 0:
+                ob = j // 5
+                if j % 5 == 0:
                     last_bank(s, ob)
-                nc.tensor.matmul(out=nums[(s, ob)][:], lhsT=evs[s][:, j % 9, P * ob:P * (ob + 1)], rhs=to_ybx[:],
-                                 is_transpose=True, start=(j % 9 == 0), stop=(j % 9 == 8))
+                nc.tensor.matmul(out=nums[(s, ob)][:], lhsT=evs[s][:, (0, 1, 2, 3, 8)[j % 5], P * ob:P * (ob + 1)], rhs=to_ybx[:],
+                                 is_transpose=True, start=(j % 5 == 0), stop=(j % 5 == 4))
             else:
                 if j == 0:
                     num = psm.tile([P, 4, P], F32, name="num", tag="num", bufs=1)
@@ -329,7 +329,7 @@ def tile_merge_pa_kernel(tc, x, w_c1, b_c1, w_q, w_k, w_v, bn_gamma, bn_beta, pr
                 pe_list.extend([("k", s + 1, AHEAD + j) for j in range(LATE)])
         for ob in range(4):
             pe_list.extend([("G", STEPS - 2, 6 * ob + j) for j in range(6)])
-            pe_list.extend([("G", STEPS - 1, 9 * ob + j) for j in range(9)])
+            pe_list.extend([("G", STEPS - 1, 5 * ob + j) for j in range(5)])
 
         done = set()
         pos = [0]
@@ -640,6 +640,9 @@ def tile_merge_pa_kernel(tc, x, w_c1, b_c1, w_q, w_k, w_v, bn_gamma, bn_beta, pr
         log_den(STEPS - 2)
         exp_minus_log(STEPS - 2)
         weigh(STEPS - 1, 0, 9)
+        ev7 = evs[STEPS - 1]
+        for c in (slice(0, 256), slice(256, 512)):
+            nc.vector.tensor_tensor(out=ev7[:, 0:4, c], in0=ev7[:, 0:4, c], in1=ev7[:, 4:8, c], op=ALU.add)
         log_den(STEPS - 1)
         exp_minus_log(STEPS - 1)
         moments(STEPS - 4, 6, 8)
@@ -659,7 +662,7 @@ def tile_merge_pa_kernel(tc, x, w_c1, b_c1, w_q, w_k, w_v, bn_gamma, bn_beta, pr
             return t[:, ob:ob + 1]
 
         def divide_block(s, ob):
-            pump_to(("G", s, 6 * ob + 5 if s == STEPS - 2 else 9 * ob + 8))
+            pump_to(("G", s, 6 * ob + 5 if s == STEPS - 2 else 5 * ob + 4))
             nc.vector.tensor_tensor(out=att[:, ob, P * s:P * (s + 1)], in0=nums[(s, ob)][:], in1=rds[s][:, ob, :], op=ALU.mult)
 
         def last_sum(ob):

@@ -109,10 +109,10 @@ def tile_merge_pa_kernel(tc, x, w_c1, b_c1, w_q, w_k, w_v, bn_gamma, bn_beta, pr
             yst = keep.tile([P, NPIX + 2 * ROW], U8, name="y_scales%d" % d, align_bytes=64)
             if d == 1:
                 for c0 in (0, ROW + NPIX):
-                    nc.vector.memset(yct[:, c0:c0 + ROW], 0)
+                    nc.gpsimd.memset(yct[:, c0:c0 + ROW].bitcast(F32), 0.0)
             else:
-                nc.vector.memset(yct[:], 0)
-            nc.vector.memset(yst[:].bitcast(I32), 0)
+                nc.gpsimd.memset(yct[:].bitcast(F32), 0.0)
+            nc.gpsimd.memset(yst[:].bitcast(F32), 0.0)
             y_codes.append(yct)
             y_scales.append(yst)
 
@@ -515,6 +515,10 @@ def tile_merge_pa_kernel(tc, x, w_c1, b_c1, w_q, w_k, w_v, bn_gamma, bn_beta, pr
             nc.scalar.activation(out=lg[:], in_=dens[s][:], func=ACT.Abs_reciprocal_sqrt)
             lgs[s] = lg
 
+        def root_of_last_den(s):
+            pump_to(("F", s, 35))
+            nc.scalar.activation(out=lg_end[:, :, s - (STEPS - 2), :], in_=dens[s][:], func=ACT.Abs_reciprocal_sqrt)
+
         def exp_minus_log(s):
             rd = main.tile([P, 4, P], F32, name="rd", tag="rd")
             nc.scalar.activation(out=rd[:], in_=lgs[s][:], func=ACT.Square)
@@ -615,10 +619,12 @@ def tile_merge_pa_kernel(tc, x, w_c1, b_c1, w_q, w_k, w_v, bn_gamma, bn_beta, pr
                 one_over_den(s - 2)
             if s == 3:
                 nc.scalar.activation(out=neg_pivot[:], in_=att[:, :, 0], func=ACT.Copy, scale=-1.0)
+                nc.scalar.activation(out=msums[:, 0, :, PAIRS], in_=att[:, :, 0], func=ACT.Copy, scale=-2.0 * P)
                 nc.scalar.activation(out=one_minus_a[:], in_=a_bf[:], func=ACT.Identity, bias=1.0, scale=-1.0)
                 nc.scalar.copy(out=gam_f[:], in_=gam_bf[:])
             if ok(s - 3) and (s - 3) % 2 == 1:
                 moments(s - 4)
+        lg_end = keep.tile([P, 4, 2, P], F32, name="lg_end")
         neg_m = main.tile([P, 512], F32, name="neg_m", tag="m")
         nc.scalar.activation(out=neg_m[:], in_=ms[STEPS - 1][:], func=ACT.Copy, scale=-1.0)
         z_last = zs[STEPS - 1]
@@ -637,14 +643,12 @@ def tile_merge_pa_kernel(tc, x, w_c1, b_c1, w_q, w_k, w_v, bn_gamma, bn_beta, pr
         exps(STEPS - 1, 1)
         moments(STEPS - 4, 3, 6)
         exps(STEPS - 1, 2)
-        log_den(STEPS - 2)
-        exp_minus_log(STEPS - 2)
+        root_of_last_den(STEPS - 2)
         weigh(STEPS - 1, 0, 9)
         ev7 = evs[STEPS - 1]
         for c in (slice(0, 256), slice(256, 512)):
             nc.vector.tensor_tensor(out=ev7[:, 0:4, c], in0=ev7[:, 0:4, c], in1=ev7[:, 4:8, c], op=ALU.add)
-        log_den(STEPS - 1)
-        exp_minus_log(STEPS - 1)
+        root_of_last_den(STEPS - 1)
         moments(STEPS - 4, 6, 8)
 
         last = slice(P * (STEPS - 2), NPIX)
@@ -661,14 +665,19 @@ def tile_merge_pa_kernel(tc, x, w_c1, b_c1, w_q, w_k, w_v, bn_gamma, bn_beta, pr
         def col(t, ob):
             return t[:, ob:ob + 1]
 
+        part = {}
+
         def divide_block(s, ob):
             pump_to(("G", s, 6 * ob + 5 if s == STEPS - 2 else 5 * ob + 4))
-            nc.vector.tensor_tensor(out=att[:, ob, P * s:P * (s + 1)], in0=nums[(s, ob)][:], in1=rds[s][:, ob, :], op=ALU.mult)
+            if ob not in part:
+                once = main.tile([P, 2, P], F32, name="once", tag="once")
+                part[ob] = once
+            nc.vector.tensor_tensor(out=part[ob][:, s - (STEPS - 2), :], in0=nums[(s, ob)][:], in1=lg_end[:, ob, s - (STEPS - 2), :], op=ALU.mult)
 
         def last_sum(ob):
-            junk_v = main.tile([P, 2 * P], F32, name="junk_v", tag="junk_v")
-            nc.vector.tensor_scalar(out=junk_v[:], in0=att[:, ob, last], scalar1=col(neg_pivot, ob), scalar2=None,
-                                    op0=ALU.add, op1=ALU.add, accum_out=msums[:, 0, ob, PAIRS - 1:PAIRS])
+            nc.vector.scalar_tensor_tensor(out=att[:, ob, last], in0=part[ob][:].rearrange("p s n -> p (s n)"), scalar=1.0,
+                                           in1=lg_end[:, ob].rearrange("p s n -> p (s n)"), op0=ALU.mult, op1=ALU.mult,
+                                           accum_out=msums[:, 0, ob, PAIRS - 1:PAIRS])
 
         def last_squares(ob):
             junk = main.tile([P, 2 * P], F32, name="junk2", tag="junk2")
@@ -717,29 +726,29 @@ def tile_merge_pa_kernel(tc, x, w_c1, b_c1, w_q, w_k, w_v, bn_gamma, bn_beta, pr
         B7 = STEPS - 1
         divide_block(B6, 0)
         divide_block(B7, 0)
-        last_squares(0)
         last_sum(0)
+        last_squares(0)
         divide_block(B6, 1)
         divide_block(B7, 1)
         totals(0)
         statistics(0)
-        last_squares(1)
         last_sum(1)
+        last_squares(1)
         normalise(0)
         divide_block(B6, 2)
         divide_block(B7, 2)
         totals(1)
         statistics(1)
-        last_squares(2)
         last_sum(2)
+        last_squares(2)
         normalise(1)
         minus_part(0)
         divide_block(B6, 3)
         divide_block(B7, 3)
         totals(2)
         statistics(2)
-        last_squares(3)
         last_sum(3)
+        last_squares(3)
         prelu_and_store(0)
         normalise(2)
         minus_part(1)

@@ -1,3 +1,4 @@
+import math
 from contextlib import ExitStack
 
 import concourse.mybir as mybir
@@ -33,6 +34,15 @@ CENTRE = 4
 AROUND = (0, 1, 2, 3, 5, 6, 7, 8)
 OFFSET_OF_SLOT = AROUND + (CENTRE,)
 GROUPS = ((0, 3), (3, 6), (6, 8))
+LAST = STEPS - 1
+LATE_Q = (0, 2)
+Y_ROWS = 19
+OWN_ROWS = 14
+INNER_ROWS = 16
+LAST_WINDOWS = ((INNER_ROWS, 0), (INNER_ROWS, 1), (INNER_ROWS, 2), (OWN_ROWS, 0), (OWN_ROWS, 2))
+OUTSIDE = 5
+LAST_EXPS = (8, 0, 1, 2, 3, 4, OUTSIDE)
+LAST_PRODUCTS = (0, 1, 2, 3, 4, 8)
 
 FLOPS = 4 * 2 * 512 * 512 * 1024
 
@@ -105,12 +115,9 @@ def tile_merge_pa_kernel(tc, x, w_c1, b_c1, w_q, w_k, w_v, bn_gamma, bn_beta, pr
         y_codes = []
         y_scales = []
         for d in range(3):
-            yct = keep.tile([P, NPIX + 2 * ROW], I32, name="y_codes%d" % d, align_bytes=64)
-            yst = keep.tile([P, NPIX + 2 * ROW], U8, name="y_scales%d" % d, align_bytes=64)
-            if d == 1:
-                for c0 in (0, ROW + NPIX):
-                    nc.gpsimd.memset(yct[:, c0:c0 + ROW].bitcast(F32), 0.0)
-            else:
+            yct = keep.tile([P, Y_ROWS * ROW], I32, name="y_codes%d" % d, align_bytes=64)
+            yst = keep.tile([P, Y_ROWS * ROW], U8, name="y_scales%d" % d, align_bytes=64)
+            if d != 1:
                 nc.gpsimd.memset(yct[:].bitcast(F32), 0.0)
             nc.gpsimd.memset(yst[:].bitcast(F32), 0.0)
             y_codes.append(yct)
@@ -190,8 +197,14 @@ def tile_merge_pa_kernel(tc, x, w_c1, b_c1, w_q, w_k, w_v, bn_gamma, bn_beta, pr
                     k_ps = psm.tile([P, 512], F32, name="k_lent", tag="den", bufs=1)
                 else:
                     k_ps = psm.tile([P, 512], F32, name="k_ps", tag="k_ps", bufs=3)
-                conv(k_ps[:], s, AROUND[j], W_K, True, False)
-                conv(k_ps[:], s, CENTRE, W_KN, False, True)
+                if s < LAST:
+                    conv(k_ps[:], s, AROUND[j], W_K, True, False)
+                    conv(k_ps[:], s, CENTRE, W_KN, False, True)
+                elif j < OUTSIDE:
+                    window(k_ps[:], LAST_WINDOWS[j][0], LAST_WINDOWS[j][1], W_K, True, False)
+                    window(k_ps[:], OWN_ROWS, 1, W_KN, False, True)
+                else:
+                    window(k_ps[:], OWN_ROWS, 1, W_KN, True, True)
                 banks[tok] = k_ps
             elif kind == "d":
                 idle = psm.tile([P, 512], F32, name="idle", tag="num", bufs=1)
@@ -248,7 +261,12 @@ def tile_merge_pa_kernel(tc, x, w_c1, b_c1, w_q, w_k, w_v, bn_gamma, bn_beta, pr
                     else:
                         den = psm.tile([P, 4, P], F32, name="den", tag="den", bufs=1)
                     dens[s] = den
-                add_up(dens[s], zs[s], j)
+                if s == LAST:
+                    n = len(LAST_EXPS)
+                    nc.tensor.matmul(out=dens[s][:, j // n, :], lhsT=zs[s][:, LAST_EXPS[j % n], P * (j // n):P * (j // n + 1)],
+                                     rhs=to_ybx[:], is_transpose=True, start=(j % n == 0), stop=(j % n == n - 1))
+                else:
+                    add_up(dens[s], zs[s], j)
             elif kind == "G" and s == STEPS - 2:
                 ob = j // 6
                 if j % 6 == 0:
@@ -257,11 +275,11 @@ def tile_merge_pa_kernel(tc, x, w_c1, b_c1, w_q, w_k, w_v, bn_gamma, bn_beta, pr
                 nc.tensor.matmul(out=nums[(s, ob)][:], lhsT=term[:, P * ob:P * (ob + 1)], rhs=to_ybx[:],
                                  is_transpose=True, start=(j % 6 == 0), stop=(j % 6 == 5))
             elif kind == "G" and s == STEPS - 1:
-                ob = j // 5
-                if j % 5 == 0:
+                ob = j // 6
+                if j % 6 == 0:
                     last_bank(s, ob)
-                nc.tensor.matmul(out=nums[(s, ob)][:], lhsT=evs[s][:, (0, 1, 2, 3, 8)[j % 5], P * ob:P * (ob + 1)], rhs=to_ybx[:],
-                                 is_transpose=True, start=(j % 5 == 0), stop=(j % 5 == 4))
+                nc.tensor.matmul(out=nums[(s, ob)][:], lhsT=evs[s][:, LAST_PRODUCTS[j % 6], P * ob:P * (ob + 1)], rhs=to_ybx[:],
+                                 is_transpose=True, start=(j % 6 == 0), stop=(j % 6 == 5))
             else:
                 if j == 0:
                     num = psm.tile([P, 4, P], F32, name="num", tag="num", bufs=1)
@@ -270,6 +288,9 @@ def tile_merge_pa_kernel(tc, x, w_c1, b_c1, w_q, w_k, w_v, bn_gamma, bn_beta, pr
 
         def products(a):
             todo = []
+            if a == LAST:
+                return ([(("v", INNER_ROWS, d), a, d) for d in range(3)]
+                        + [(("v", OWN_ROWS, 0), a, 3), (("v", OWN_ROWS, 2), a, 4), (("v", OWN_ROWS, 1), a, 8)])
             if a <= SHARE_FROM:
                 todo.extend([(("u", 2 * a - 1, d), a, d) for d in range(3)])
             todo.append((("v", 2 * a, 0), a, 3))
@@ -277,7 +298,7 @@ def tile_merge_pa_kernel(tc, x, w_c1, b_c1, w_q, w_k, w_v, bn_gamma, bn_beta, pr
             todo.append((("v", 2 * a, 1), a, 8))
             for d in range(3):
                 todo.append((("v", 2 * a + 1, d), a, 5 + d))
-                if ok(a + 1) and a >= SHARE_FROM:
+                if a + 1 < LAST and a >= SHARE_FROM:
                     todo.append((("v", 2 * a + 1, d), a + 1, d))
             return todo
 
@@ -290,6 +311,12 @@ def tile_merge_pa_kernel(tc, x, w_c1, b_c1, w_q, w_k, w_v, bn_gamma, bn_beta, pr
 
         lent_to_v = [v_banks(a)[3] for a in range(STEPS)]
 
+        def scores_of(s):
+            return OUTSIDE + 1 if s == LAST else 8
+
+        def den_terms(s):
+            return 4 * len(LAST_EXPS) if s == LAST else 36
+
         def on_pe(pc):
             return [("h", pc, b) for b in range(NB) if (pc, b) not in HAAR_ON_VECTOR]
 
@@ -299,8 +326,8 @@ def tile_merge_pa_kernel(tc, x, w_c1, b_c1, w_q, w_k, w_v, bn_gamma, bn_beta, pr
         for s in range(STEPS + 2):
             a = s - 2
             if ok(s):
-                pe_list.extend([("k", s, j) for j in range(AHEAD if s == 0 else AHEAD + LATE, 8)])
-            if ok(s + 1):
+                pe_list.extend([("k", s, j) for j in range(AHEAD if s == 0 else AHEAD + LATE, scores_of(s))])
+            if ok(s + 1) and s not in LATE_Q:
                 pe_list.append(("q", s + 1, 0))
             if s == 0:
                 pe_list.extend([("C", 1, t) for t in range(4)] + [("w", W_V, 0), ("w", W_V, 1)] + on_pe(2))
@@ -308,7 +335,7 @@ def tile_merge_pa_kernel(tc, x, w_c1, b_c1, w_q, w_k, w_v, bn_gamma, bn_beta, pr
                 pe_list.extend([("C", 2, t) for t in range(4)])
             vb = v_banks(a)[3 if a >= EARLY_FROM else 0:] if ok(a) else []
             early = v_banks(a + 1)[:3] if ok(a + 1) and a + 1 >= EARLY_FROM else []
-            den_sums = [("F", a, i) for i in range(36)] if ok(a) else []
+            den_sums = [("F", a, i) for i in range(den_terms(a))] if ok(a) else []
             num_sums = [("G", a, i) for i in range(36)] if ok(a) and a < STEPS - 2 else []
             if a == STEPS - 2:
                 pe_list.extend(den_sums)
@@ -320,6 +347,8 @@ def tile_merge_pa_kernel(tc, x, w_c1, b_c1, w_q, w_k, w_v, bn_gamma, bn_beta, pr
                 pe_list.extend(vb[:3] + den_sums[:9] + vb[3:5] + den_sums[9:18] + vb[5:])
             else:
                 pe_list.extend(den_sums[:18] + vb)
+            if s in LATE_Q:
+                pe_list.append(("q", s + 1, 0))
             if ok(s + 1):
                 pe_list.extend([("k", s + 1, j) for j in range(AHEAD)])
             pe_list.extend(den_sums[18:])
@@ -329,7 +358,7 @@ def tile_merge_pa_kernel(tc, x, w_c1, b_c1, w_q, w_k, w_v, bn_gamma, bn_beta, pr
                 pe_list.extend([("k", s + 1, AHEAD + j) for j in range(LATE)])
         for ob in range(4):
             pe_list.extend([("G", STEPS - 2, 6 * ob + j) for j in range(6)])
-            pe_list.extend([("G", STEPS - 1, 5 * ob + j) for j in range(5)])
+            pe_list.extend([("G", STEPS - 1, 6 * ob + j) for j in range(6)])
 
         done = set()
         pos = [0]
@@ -420,17 +449,22 @@ def tile_merge_pa_kernel(tc, x, w_c1, b_c1, w_q, w_k, w_v, bn_gamma, bn_beta, pr
         def quant_y(pc):
             p0 = ROW * PIECES[pc][0]
             n = ROW * PIECES[pc][1]
-            nc.vector.quantize_mx(out=y_codes[1][:, ROW + p0:ROW + p0 + n].bitcast(FP8X4),
-                                  scales=y_scales[1][:, ROW + p0:ROW + p0 + n],
+            nc.vector.quantize_mx(out=y_codes[1][:, p0:p0 + n].bitcast(FP8X4),
+                                  scales=y_scales[1][:, p0:p0 + n],
                                   in_=y_mid[:].rearrange("p c j -> p (c j)")[:, 4 * p0:4 * (p0 + n)])
 
         code_rows = [t[:].rearrange("p (r c) -> p r c", c=ROW) for t in y_codes]
         scale_rows = [t[:].bitcast(I32).rearrange("p (r c) -> p r c", c=ROW // 4) for t in y_scales]
 
         def move_y(pc):
-            r0 = 1 + PIECES[pc][0]
+            r0 = PIECES[pc][0]
             r1 = r0 + PIECES[pc][1]
             w = ROW // 4
+            if r1 == 16:
+                for rows in (code_rows[1], scale_rows[1]):
+                    nc.vector.tensor_copy(out=rows[:, 16:19:2, :], in_=rows[:, 0:2, :])
+                    nc.vector.tensor_copy(out=rows[:, 17, :], in_=rows[:, 14, :])
+                r1 = Y_ROWS
             nc.vector.tensor_copy(out=code_rows[0][:, r0:r1, NB:ROW], in_=code_rows[1][:, r0:r1, 0:ROW - NB])
             nc.vector.tensor_copy(out=code_rows[2][:, r0:r1, 0:ROW - NB], in_=code_rows[1][:, r0:r1, NB:ROW])
             nc.vector.tensor_copy(out=scale_rows[0][:, r0:r1, 1:w], in_=scale_rows[1][:, r0:r1, 0:w - 1])
@@ -459,16 +493,18 @@ def tile_merge_pa_kernel(tc, x, w_c1, b_c1, w_q, w_k, w_v, bn_gamma, bn_beta, pr
         def tree_in_halves(s, between, on_vector=0):
             z = zs[s]
             halves = (slice(0, 256), slice(256, 512))
+            n = scores_of(s) // 2
             t1 = main.tile([P, 4, 512], F32, name="t1", tag="t1", bufs=1)
             for c in halves:
-                nc.vector.tensor_tensor(out=t1[:, :, c], in0=z[:, 0:4, c], in1=z[:, 4:8, c], op=ALU.max)
+                nc.vector.tensor_tensor(out=t1[:, 0:n, c], in0=z[:, 0:n, c], in1=z[:, n:2 * n, c], op=ALU.max)
             between()
             t2 = main.tile([P, 2, 512], F32, name="t2", tag="t2", bufs=1)
             for c in halves:
-                nc.vector.tensor_tensor(out=t2[:, :, c], in0=t1[:, 0:2, c], in1=t1[:, 2:4, c], op=ALU.max)
+                nc.vector.tensor_tensor(out=t2[:, 0:n // 2, c], in0=t1[:, 0:n // 2, c], in1=t1[:, n // 2:2 * (n // 2), c], op=ALU.max)
             m = main.tile([P, 512], F32, name="m", tag="m")
             for c in halves:
-                nc.vector.scalar_tensor_tensor(out=m[:, c], in0=t2[:, 0, c], scalar=0.0, in1=t2[:, 1, c], op0=ALU.max, op1=ALU.max)
+                other = t1[:, 2, c] if s == LAST else t2[:, 1, c]
+                nc.vector.scalar_tensor_tensor(out=m[:, c], in0=t2[:, 0, c], scalar=0.0, in1=other, op0=ALU.max, op1=ALU.max)
             ms[s] = m
             for g in range(len(GROUPS)):
                 if 3 * g < on_vector:
@@ -499,7 +535,12 @@ def tile_merge_pa_kernel(tc, x, w_c1, b_c1, w_q, w_k, w_v, bn_gamma, bn_beta, pr
             if g == 0:
                 nc.scalar.activation(out=z[:, 8, :], in_=ms[s][:], func=ACT.Exp, scale=-1.0)
             g0, g1 = GROUPS[g]
-            nc.scalar.activation(out=z[:, g0:g1, :], in_=z[:, g0:g1, :], func=ACT.Exp)
+            if s == LAST and g == 1:
+                g1 = OUTSIDE
+            if s == LAST and g == 2:
+                nc.scalar.activation(out=z[:, OUTSIDE, :], in_=z[:, OUTSIDE, :], func=ACT.Exp, bias=math.log(3.0))
+            else:
+                nc.scalar.activation(out=z[:, g0:g1, :], in_=z[:, g0:g1, :], func=ACT.Exp)
 
         def weigh(a, i0, i1):
             for tok, s, slot in products(a)[i0:i1]:
@@ -516,7 +557,7 @@ def tile_merge_pa_kernel(tc, x, w_c1, b_c1, w_q, w_k, w_v, bn_gamma, bn_beta, pr
             lgs[s] = lg
 
         def root_of_last_den(s):
-            pump_to(("F", s, 35))
+            pump_to(("F", s, den_terms(s) - 1))
             nc.scalar.activation(out=lg_end[:, :, s - (STEPS - 2), :], in_=dens[s][:], func=ACT.Abs_reciprocal_sqrt)
 
         def exp_minus_log(s):
@@ -577,32 +618,39 @@ def tile_merge_pa_kernel(tc, x, w_c1, b_c1, w_q, w_k, w_v, bn_gamma, bn_beta, pr
         haar_on_vector(1, (2, 3), True)
         scores(0, 0, AHEAD)
         for s in range(STEPS):
-            scores(s, AHEAD, 8)
+            scores(s, AHEAD, scores_of(s))
             if s == 1:
                 late_sums = haar_by_reduce(2, 2)
             if ok(s - 1):
                 exps(s - 1, 0)
-            if s > 0 and ok(s + 1):
+            if ok(s + 1) and s not in LATE_Q:
                 q_copy(s + 1)
             if s == 1:
                 halve(2, 2, late_sums[:])
             if ok(s - 3):
                 divide(s - 3)
-            if ok(s - 2):
-                weigh(s - 2, 0, 12)
             if s == 2:
+                weigh(0, 0, 4)
                 quant_y(2)
+                weigh(0, 4, 12)
+            elif ok(s - 2):
+                weigh(s - 2, 0, 12)
             if s == 0:
-                shift_by_max(s, (lambda: (quant_ll(1), q_copy(1), add_bias_on_scalar(1)()),
+                shift_by_max(s, (lambda: (quant_ll(1), add_bias_on_scalar(1)()),
                                  lambda: haar_on_vector(2, (0, 1)), lambda: quant_y(1)), 0, True)
             elif s == 1:
                 shift_by_max(s, (lambda: quant_ll(2), lambda: quant_w(W_V, g_v), nothing), 0, True)
                 scores(s + 1, 0, AHEAD)
             else:
                 tree_in_halves(s, (lambda: move_y(2)) if s == 2 else nothing, LAST_ON_VECTOR if s == STEPS - 1 else 0)
+                if s == 2:
+                    exps(1, 1)
+                    exps(1, 2)
+                    q_copy(3)
                 if ok(s + 1):
                     scores(s + 1, 0, AHEAD)
             if s == 0:
+                q_copy(1)
                 move_y(1)
                 g_v = weight_copies(W_V)
                 haar_from_pe(2)
@@ -612,7 +660,7 @@ def tile_merge_pa_kernel(tc, x, w_c1, b_c1, w_q, w_k, w_v, bn_gamma, bn_beta, pr
                 exps(0, 1)
                 weave()
                 exps(0, 2)
-            elif ok(s - 1):
+            elif ok(s - 1) and s != 2:
                 exps(s - 1, 1)
                 exps(s - 1, 2)
             if ok(s - 2):
@@ -628,7 +676,7 @@ def tile_merge_pa_kernel(tc, x, w_c1, b_c1, w_q, w_k, w_v, bn_gamma, bn_beta, pr
         neg_m = main.tile([P, 512], F32, name="neg_m", tag="m")
         nc.scalar.activation(out=neg_m[:], in_=ms[STEPS - 1][:], func=ACT.Copy, scale=-1.0)
         z_last = zs[STEPS - 1]
-        for g0, g1 in GROUPS[LAST_ON_VECTOR // 3:]:
+        for g0, g1 in ((3, OUTSIDE), (OUTSIDE, OUTSIDE + 1)):
             nc.gpsimd.tensor_tensor(out=z_last[:, g0:g1, :], in0=z_last[:, g0:g1, :],
                                     in1=neg_m[:].unsqueeze(1).to_broadcast([P, g1 - g0, 512]), op=ALU.add)
         divide(STEPS - 3)
@@ -639,15 +687,12 @@ def tile_merge_pa_kernel(tc, x, w_c1, b_c1, w_q, w_k, w_v, bn_gamma, bn_beta, pr
         ev_sums.append(ev_sum)
         ev6 = evs[STEPS - 2]
         nc.gpsimd.tensor_tensor(out=ev_sum[:], in0=ev6[:, 0:3, :], in1=ev6[:, 3:6, :], op=ALU.add)
-        weigh(STEPS - 2, 4, 9)
+        weigh(STEPS - 2, 4, 6)
         exps(STEPS - 1, 1)
         moments(STEPS - 4, 3, 6)
         exps(STEPS - 1, 2)
         root_of_last_den(STEPS - 2)
-        weigh(STEPS - 1, 0, 9)
-        ev7 = evs[STEPS - 1]
-        for c in (slice(0, 256), slice(256, 512)):
-            nc.vector.tensor_tensor(out=ev7[:, 0:4, c], in0=ev7[:, 0:4, c], in1=ev7[:, 4:8, c], op=ALU.add)
+        weigh(STEPS - 1, 0, 6)
         root_of_last_den(STEPS - 1)
         moments(STEPS - 4, 6, 8)
 
@@ -668,7 +713,7 @@ def tile_merge_pa_kernel(tc, x, w_c1, b_c1, w_q, w_k, w_v, bn_gamma, bn_beta, pr
         part = {}
 
         def divide_block(s, ob):
-            pump_to(("G", s, 6 * ob + 5 if s == STEPS - 2 else 5 * ob + 4))
+            pump_to(("G", s, 6 * ob + 5))
             if ob not in part:
                 once = main.tile([P, 2, P], F32, name="once", tag="once")
                 part[ob] = once
@@ -720,7 +765,9 @@ def tile_merge_pa_kernel(tc, x, w_c1, b_c1, w_q, w_k, w_v, bn_gamma, bn_beta, pr
             res = mid.tile([P, NPIX], F32, name="res", tag=("ll", "y_mid", "res_c", "res_d")[ob], align_bytes=64)
             nc.vector.scalar_tensor_tensor(out=res[:], in0=negs[ob][:], scalar=one_minus_a[:, 0:1], in1=ns[ob][:],
                                            op0=ALU.mult, op1=ALU.add)
-            nc.sync.dma_start(out=out_v[:, ob], in_=res[:].rearrange("p (b f) -> p b f", b=NB))
+            by_image = res[:].rearrange("p (b f) -> p b f", b=NB)
+            nc.sync.dma_start(out=out_v[:, ob, :, 16:256], in_=by_image[:, :, 0:240])
+            nc.sync.dma_start(out=out_v[:, ob, :, 0:16], in_=by_image[:, :, 240:256])
 
         B6 = STEPS - 2
         B7 = STEPS - 1

@@ -348,7 +348,8 @@ def tile_merge_pa_kernel(tc, x, w_c1, b_c1, w_q, w_k, w_v, bn_gamma, bn_beta, pr
             else:
                 pe_list.extend(den_sums[:18] + vb)
             if s in LATE_Q:
-                pe_list.append(("q", s + 1, 0))
+                pe_list.extend(den_sums[18:] + [("q", s + 1, 0)])
+                den_sums = den_sums[:18]
             if ok(s + 1):
                 pe_list.extend([("k", s + 1, j) for j in range(AHEAD)])
             pe_list.extend(den_sums[18:])
@@ -629,12 +630,10 @@ def tile_merge_pa_kernel(tc, x, w_c1, b_c1, w_q, w_k, w_v, bn_gamma, bn_beta, pr
                 halve(2, 2, late_sums[:])
             if ok(s - 3):
                 divide(s - 3)
-            if s == 2:
-                weigh(0, 0, 4)
-                quant_y(2)
-                weigh(0, 4, 12)
-            elif ok(s - 2):
+            if ok(s - 2):
                 weigh(s - 2, 0, 12)
+            if s == 2:
+                quant_y(2)
             if s == 0:
                 shift_by_max(s, (lambda: (quant_ll(1), add_bias_on_scalar(1)()),
                                  lambda: haar_on_vector(2, (0, 1)), lambda: quant_y(1)), 0, True)
@@ -763,11 +762,13 @@ def tile_merge_pa_kernel(tc, x, w_c1, b_c1, w_q, w_k, w_v, bn_gamma, bn_beta, pr
 
         def prelu_and_store(ob):
             res = mid.tile([P, NPIX], F32, name="res", tag=("ll", "y_mid", "res_c", "res_d")[ob], align_bytes=64)
-            nc.vector.scalar_tensor_tensor(out=res[:], in0=negs[ob][:], scalar=one_minus_a[:, 0:1], in1=ns[ob][:],
-                                           op0=ALU.mult, op1=ALU.add)
-            by_image = res[:].rearrange("p (b f) -> p b f", b=NB)
-            nc.sync.dma_start(out=out_v[:, ob, :, 16:256], in_=by_image[:, :, 0:240])
-            nc.sync.dma_start(out=out_v[:, ob, :, 0:16], in_=by_image[:, :, 240:256])
+            for src0, n_el, dst0 in ((0, 240, 16), (240, 16, 0)):
+                nc.vector.scalar_tensor_tensor(out=res[:].rearrange("p (b f) -> p b f", b=NB)[:, :, dst0:dst0 + n_el],
+                                               in0=negs[ob][:].rearrange("p (b f) -> p b f", b=NB)[:, :, src0:src0 + n_el],
+                                               scalar=one_minus_a[:, 0:1],
+                                               in1=ns[ob][:].rearrange("p (b f) -> p b f", b=NB)[:, :, src0:src0 + n_el],
+                                               op0=ALU.mult, op1=ALU.add)
+            nc.sync.dma_start(out=out_v[:, ob], in_=res[:].rearrange("p (b f) -> p b f", b=NB))
 
         B6 = STEPS - 2
         B7 = STEPS - 1

@@ -39,10 +39,8 @@ LATE_Q = (0, 2)
 Y_ROWS = 19
 OWN_ROWS = 14
 INNER_ROWS = 16
-LAST_WINDOWS = ((INNER_ROWS, 0), (INNER_ROWS, 1), (INNER_ROWS, 2), (OWN_ROWS, 0), (OWN_ROWS, 2))
-OUTSIDE = 5
-LAST_EXPS = (8, 0, 1, 2, 3, 4, OUTSIDE)
-LAST_PRODUCTS = (0, 1, 2, 3, 4, 8)
+LAST_WINDOWS = ((INNER_ROWS, 0), (INNER_ROWS, 1), (INNER_ROWS, 2), (OWN_ROWS, 0), (OWN_ROWS, 2), (OWN_ROWS, 1))
+LAST_EXPS = (8, 0, 1, 2, 3, 4, 5)
 
 FLOPS = 4 * 2 * 512 * 512 * 1024
 
@@ -200,11 +198,8 @@ def tile_merge_pa_kernel(tc, x, w_c1, b_c1, w_q, w_k, w_v, bn_gamma, bn_beta, pr
                 if s < LAST:
                     conv(k_ps[:], s, AROUND[j], W_K, True, False)
                     conv(k_ps[:], s, CENTRE, W_KN, False, True)
-                elif j < OUTSIDE:
-                    window(k_ps[:], LAST_WINDOWS[j][0], LAST_WINDOWS[j][1], W_K, True, False)
-                    window(k_ps[:], OWN_ROWS, 1, W_KN, False, True)
                 else:
-                    window(k_ps[:], OWN_ROWS, 1, W_KN, True, True)
+                    window(k_ps[:], LAST_WINDOWS[j][0], LAST_WINDOWS[j][1], W_K, True, True)
                 banks[tok] = k_ps
             elif kind == "d":
                 idle = psm.tile([P, 512], F32, name="idle", tag="num", bufs=1)
@@ -278,7 +273,7 @@ def tile_merge_pa_kernel(tc, x, w_c1, b_c1, w_q, w_k, w_v, bn_gamma, bn_beta, pr
                 ob = j // 6
                 if j % 6 == 0:
                     last_bank(s, ob)
-                nc.tensor.matmul(out=nums[(s, ob)][:], lhsT=evs[s][:, LAST_PRODUCTS[j % 6], P * ob:P * (ob + 1)], rhs=to_ybx[:],
+                nc.tensor.matmul(out=nums[(s, ob)][:], lhsT=evs[s][:, j % 6, P * ob:P * (ob + 1)], rhs=to_ybx[:],
                                  is_transpose=True, start=(j % 6 == 0), stop=(j % 6 == 5))
             else:
                 if j == 0:
@@ -289,8 +284,7 @@ def tile_merge_pa_kernel(tc, x, w_c1, b_c1, w_q, w_k, w_v, bn_gamma, bn_beta, pr
         def products(a):
             todo = []
             if a == LAST:
-                return ([(("v", INNER_ROWS, d), a, d) for d in range(3)]
-                        + [(("v", OWN_ROWS, 0), a, 3), (("v", OWN_ROWS, 2), a, 4), (("v", OWN_ROWS, 1), a, 8)])
+                return [(("v", LAST_WINDOWS[j][0], LAST_WINDOWS[j][1]), a, j) for j in range(len(LAST_WINDOWS))]
             if a <= SHARE_FROM:
                 todo.extend([(("u", 2 * a - 1, d), a, d) for d in range(3)])
             todo.append((("v", 2 * a, 0), a, 3))
@@ -312,7 +306,7 @@ def tile_merge_pa_kernel(tc, x, w_c1, b_c1, w_q, w_k, w_v, bn_gamma, bn_beta, pr
         lent_to_v = [v_banks(a)[3] for a in range(STEPS)]
 
         def scores_of(s):
-            return OUTSIDE + 1 if s == LAST else 8
+            return len(LAST_WINDOWS) if s == LAST else 8
 
         def den_terms(s):
             return 4 * len(LAST_EXPS) if s == LAST else 36
@@ -534,14 +528,12 @@ def tile_merge_pa_kernel(tc, x, w_c1, b_c1, w_q, w_k, w_v, bn_gamma, bn_beta, pr
         def exps(s, g):
             z = zs[s]
             if g == 0:
-                nc.scalar.activation(out=z[:, 8, :], in_=ms[s][:], func=ACT.Exp, scale=-1.0)
+                if s == LAST:
+                    nc.scalar.activation(out=z[:, 8, :], in_=ms[s][:], func=ACT.Exp, scale=-1.0, bias=math.log(3.0))
+                else:
+                    nc.scalar.activation(out=z[:, 8, :], in_=ms[s][:], func=ACT.Exp, scale=-1.0)
             g0, g1 = GROUPS[g]
-            if s == LAST and g == 1:
-                g1 = OUTSIDE
-            if s == LAST and g == 2:
-                nc.scalar.activation(out=z[:, OUTSIDE, :], in_=z[:, OUTSIDE, :], func=ACT.Exp, bias=math.log(3.0))
-            else:
-                nc.scalar.activation(out=z[:, g0:g1, :], in_=z[:, g0:g1, :], func=ACT.Exp)
+            nc.scalar.activation(out=z[:, g0:g1, :], in_=z[:, g0:g1, :], func=ACT.Exp)
 
         def weigh(a, i0, i1):
             for tok, s, slot in products(a)[i0:i1]:
@@ -675,7 +667,7 @@ def tile_merge_pa_kernel(tc, x, w_c1, b_c1, w_q, w_k, w_v, bn_gamma, bn_beta, pr
         neg_m = main.tile([P, 512], F32, name="neg_m", tag="m")
         nc.scalar.activation(out=neg_m[:], in_=ms[STEPS - 1][:], func=ACT.Copy, scale=-1.0)
         z_last = zs[STEPS - 1]
-        for g0, g1 in ((3, OUTSIDE), (OUTSIDE, OUTSIDE + 1)):
+        for g0, g1 in GROUPS[1:2]:
             nc.gpsimd.tensor_tensor(out=z_last[:, g0:g1, :], in0=z_last[:, g0:g1, :],
                                     in1=neg_m[:].unsqueeze(1).to_broadcast([P, g1 - g0, 512]), op=ALU.add)
         divide(STEPS - 3)
@@ -689,7 +681,6 @@ def tile_merge_pa_kernel(tc, x, w_c1, b_c1, w_q, w_k, w_v, bn_gamma, bn_beta, pr
         weigh(STEPS - 2, 4, 6)
         exps(STEPS - 1, 1)
         moments(STEPS - 4, 3, 6)
-        exps(STEPS - 1, 2)
         root_of_last_den(STEPS - 2)
         weigh(STEPS - 1, 0, 6)
         root_of_last_den(STEPS - 1)

@@ -562,10 +562,16 @@ def tile_merge_pa_kernel(tc, x, w_c1, b_c1, w_q, w_k, w_v, bn_gamma, bn_beta, pr
             log_den(s)
             exp_minus_log(s)
 
-        def divide(s):
+        def divide(s, on_vector=4):
             pump_to(("G", s, 35))
             cols = slice(P * s, P * (s + 1))
-            nc.vector.tensor_tensor(out=att[:, :, cols], in0=nums[s][:], in1=rds[s][:], op=ALU.mult)
+            if on_vector < 4:
+                num_sb = main.tile([P, 4 - on_vector, P], F32, name="num_sb", tag="num_sb")
+                nc.scalar.copy(out=num_sb[:], in_=nums[s][:, on_vector:4, :])
+            nc.vector.tensor_tensor(out=att[:, 0:on_vector, cols], in0=nums[s][:, 0:on_vector, :], in1=rds[s][:, 0:on_vector, :],
+                                    op=ALU.mult)
+            if on_vector < 4:
+                nc.gpsimd.tensor_tensor(out=att[:, on_vector:4, cols], in0=num_sb[:], in1=rds[s][:, on_vector:4, :], op=ALU.mult)
 
         def moments(s, first=0, end=8):
             cols = slice(P * s, P * (s + 2))
@@ -612,6 +618,8 @@ def tile_merge_pa_kernel(tc, x, w_c1, b_c1, w_q, w_k, w_v, bn_gamma, bn_beta, pr
         scores(0, 0, AHEAD)
         for s in range(STEPS):
             scores(s, AHEAD, scores_of(s))
+            if ok(s - 3):
+                divide(s - 3, 2)
             if s == 1:
                 late_sums = haar_by_reduce(2, 2)
             if ok(s - 1):
@@ -620,8 +628,6 @@ def tile_merge_pa_kernel(tc, x, w_c1, b_c1, w_q, w_k, w_v, bn_gamma, bn_beta, pr
                 q_copy(s + 1)
             if s == 1:
                 halve(2, 2, late_sums[:])
-            if ok(s - 3):
-                divide(s - 3)
             if ok(s - 2):
                 weigh(s - 2, 0, 12)
             if s == 2:

@@ -25,7 +25,7 @@ WARM_UP = 4
 EARLY_FROM = 1
 FIRST_LENT = 2
 LATE = 2
-LAST_BANKS = (("num", 1), ("k_ps", 3), ("k_ps", 3), ("v_ps", 3), ("v_ps", 3), ("v_ps", 3), ("den", 1), ("k_ps", 3))
+LAST_BANKS = (("k_ps", 3), ("k_ps", 3), ("k_ps", 3), ("v_ps", 3), ("v_ps", 3), ("v_ps", 3), ("den", 1), ("num", 1))
 LAST_ON_VECTOR = 3
 PIECES = ((0, 4), (4, 4), (8, 8))
 HAAR_ON_VECTOR = ((0, 0), (0, 1), (1, 2), (1, 3), (2, 0), (2, 1), (2, 2))
@@ -75,9 +75,9 @@ def tile_merge_pa_kernel(tc, x, w_c1, b_c1, w_q, w_k, w_v, bn_gamma, bn_beta, pr
                                   in_=x[b].rearrange("(p j) h w -> p j (h w)", j=4)[:, :, ROW * row0:ROW * (row0 + nr)])
 
         bias_bf = keep.tile([P, 4], BF16, name="bias_bf")
-        nc.sync.dma_start(out=bias_bf[:], in_=b_c1.rearrange("(p t) -> p t", t=4))
         load_w(W_C1)
         load_x(0)
+        nc.sync.dma_start(out=bias_bf[:], in_=b_c1.rearrange("(p t) -> p t", t=4))
         load_w(W_Q)
         load_w(W_K, 2)
         load_x(1)
@@ -206,7 +206,9 @@ def tile_merge_pa_kernel(tc, x, w_c1, b_c1, w_q, w_k, w_v, bn_gamma, bn_beta, pr
                 nc.tensor.matmul_mx(out=idle[:], lhsT=w_codes[W_KN][:, 0:P].bitcast(FP8X4), lhsT_scale=w_scales[W_KN][:, 0:P],
                                     rhs=w_codes[W_KN][:].bitcast(FP8X4), rhs_scale=w_scales[W_KN][:], start=True, stop=True)
             elif kind in ("v", "u"):
-                if tok in lent_to_v:
+                if tok in in_k_banks:
+                    v_ps = psm.tile([P, 512], F32, name="v_in_k", tag="k_ps", bufs=3)
+                elif tok in lent_to_v:
                     v_ps = psm.tile([P, 512], F32, name="v_lent", tag="num", bufs=1)
                 else:
                     v_ps = psm.tile([P, 512], F32, name="v_ps", tag="v_ps", bufs=3)
@@ -252,7 +254,7 @@ def tile_merge_pa_kernel(tc, x, w_c1, b_c1, w_q, w_k, w_v, bn_gamma, bn_beta, pr
             elif kind == "F":
                 if j == 0:
                     if s == STEPS - 1:
-                        den = psm.tile([P, 4, P], F32, name="den_last", tag="k_ps", bufs=3)
+                        den = psm.tile([P, 4, P], F32, name="den_last", tag="num", bufs=1)
                     else:
                         den = psm.tile([P, 4, P], F32, name="den", tag="den", bufs=1)
                     dens[s] = den
@@ -303,7 +305,8 @@ def tile_merge_pa_kernel(tc, x, w_c1, b_c1, w_q, w_k, w_v, bn_gamma, bn_beta, pr
                     toks.append(tok)
             return toks
 
-        lent_to_v = [v_banks(a)[3] for a in range(STEPS)]
+        lent_to_v = [v_banks(a)[3] for a in range(STEPS - 2)]
+        in_k_banks = v_banks(STEPS - 2)[3:] + v_banks(STEPS - 1)[3:]
 
         def scores_of(s):
             return len(LAST_WINDOWS) if s == LAST else 8
@@ -332,11 +335,16 @@ def tile_merge_pa_kernel(tc, x, w_c1, b_c1, w_q, w_k, w_v, bn_gamma, bn_beta, pr
             den_sums = [("F", a, i) for i in range(den_terms(a))] if ok(a) else []
             num_sums = [("G", a, i) for i in range(36)] if ok(a) and a < STEPS - 2 else []
             if a == STEPS - 2:
-                pe_list.extend(den_sums)
+                pe_list.extend(vb + den_sums)
+                vb = []
                 den_sums = []
             if a == STEPS - 1:
                 pe_list.extend(vb)
                 vb = []
+            if s == STEPS - 1:
+                pe_list.extend(den_sums + vb)
+                vb = []
+                den_sums = []
             if ok(a) and a < EARLY_FROM:
                 pe_list.extend(vb[:3] + den_sums[:9] + vb[3:5] + den_sums[9:18] + vb[5:])
             else:
@@ -619,7 +627,7 @@ def tile_merge_pa_kernel(tc, x, w_c1, b_c1, w_q, w_k, w_v, bn_gamma, bn_beta, pr
         for s in range(STEPS):
             scores(s, AHEAD, scores_of(s))
             if ok(s - 3):
-                divide(s - 3, 2)
+                divide(s - 3, 2 if s < STEPS - 1 else 4)
             if s == 1:
                 late_sums = haar_by_reduce(2, 2)
             if ok(s - 1):
@@ -658,9 +666,11 @@ def tile_merge_pa_kernel(tc, x, w_c1, b_c1, w_q, w_k, w_v, bn_gamma, bn_beta, pr
                 weave()
                 exps(0, 2)
             elif ok(s - 1) and s != 2:
+                if s == STEPS - 1:
+                    one_over_den(s - 2)
                 exps(s - 1, 1)
                 exps(s - 1, 2)
-            if ok(s - 2):
+            if ok(s - 2) and s < STEPS - 1:
                 one_over_den(s - 2)
             if s == 3:
                 nc.scalar.activation(out=neg_pivot[:], in_=att[:, :, 0], func=ACT.Copy, scale=-1.0)
@@ -686,11 +696,10 @@ def tile_merge_pa_kernel(tc, x, w_c1, b_c1, w_q, w_k, w_v, bn_gamma, bn_beta, pr
         nc.gpsimd.tensor_tensor(out=ev_sum[:], in0=ev6[:, 0:3, :], in1=ev6[:, 3:6, :], op=ALU.add)
         weigh(STEPS - 2, 4, 6)
         exps(STEPS - 1, 1)
-        moments(STEPS - 4, 3, 6)
         root_of_last_den(STEPS - 2)
         weigh(STEPS - 1, 0, 6)
         root_of_last_den(STEPS - 1)
-        moments(STEPS - 4, 6, 8)
+        moments(STEPS - 4, 3, 6)
 
         last = slice(P * (STEPS - 2), NPIX)
         tot = keep.tile([P, 2, 4], F32, name="tot")
@@ -702,6 +711,7 @@ def tile_merge_pa_kernel(tc, x, w_c1, b_c1, w_q, w_k, w_v, bn_gamma, bn_beta, pr
         out_v = out.rearrange("b (c r) h w -> c r b (h w)", r=4)
         ns = {}
         negs = {}
+        ress = {}
 
         def col(t, ob):
             return t[:, ob:ob + 1]
@@ -744,28 +754,40 @@ def tile_merge_pa_kernel(tc, x, w_c1, b_c1, w_q, w_k, w_v, bn_gamma, bn_beta, pr
                 n = main.tile([P, NPIX], F32, name="n", tag="z", bufs=3)
             else:
                 n = main.tile([P, NPIX], F32, name="n_last", tag="ev", bufs=2)
-            nc.scalar.activation(out=n[:].rearrange("p (b y x) -> p b y x", b=NB, x=16),
-                                 in_=att[:, ob, :].rearrange("p (y b x) -> p b y x", b=NB, x=16),
-                                 func=ACT.Identity, bias=col(shift, ob), scale=col(gain, ob))
             ns[ob] = n
+            if ob < 3:
+                normalise_images(ob, 0, NB)
 
-        def minus_part(ob, on_scalar=False):
+        def normalise_images(ob, b0, b1):
+            nc.scalar.activation(out=ns[ob][:].rearrange("p (b y x) -> p b y x", b=NB, x=16)[:, b0:b1],
+                                 in_=att[:, ob, :].rearrange("p (y b x) -> p b y x", b=NB, x=16)[:, b0:b1],
+                                 func=ACT.Identity, bias=col(shift, ob), scale=col(gain, ob))
+
+        def minus_part(ob):
             neg = main.tile([P, NPIX], F32, name="neg", tag=("t1", "t2")[ob % 2], bufs=1)
-            if on_scalar:
-                nc.scalar.activation(out=neg[:], in_=ns[ob][:], func=ACT.Relu, scale=-1.0)
-            else:
-                nc.vector.tensor_scalar(out=neg[:], in0=ns[ob][:], scalar1=-1.0, scalar2=0.0, op0=ALU.mult, op1=ALU.max)
+            nc.vector.tensor_scalar(out=neg[:], in0=ns[ob][:], scalar1=-1.0, scalar2=0.0, op0=ALU.mult, op1=ALU.max)
             negs[ob] = neg
 
-        def prelu_and_store(ob):
-            res = mid.tile([P, NPIX], F32, name="res", tag=("ll", "y_mid", "res_c", "res_d")[ob], align_bytes=64)
+        def last_parts():
+            neg = main.tile([P, NPIX], F32, name="neg_last", tag="t2", bufs=1)
+            negs[3] = neg
+            half = NPIX // 2
+            for h in range(2):
+                normalise_images(3, 2 * h, 2 * h + 2)
+                nc.scalar.activation(out=neg[:, half * h:half * (h + 1)], in_=ns[3][:, half * h:half * (h + 1)], func=ACT.Relu, scale=-1.0)
+
+        def prelu_and_store(ob, b0=0, b1=NB):
+            if b0 == 0:
+                res = mid.tile([P, NPIX], F32, name="res", tag=("ll", "y_mid", "res_c", "res_d")[ob], align_bytes=64)
+                ress[ob] = res
+            res = ress[ob]
             for src0, n_el, dst0 in ((0, 240, 16), (240, 16, 0)):
-                nc.vector.scalar_tensor_tensor(out=res[:].rearrange("p (b f) -> p b f", b=NB)[:, :, dst0:dst0 + n_el],
-                                               in0=negs[ob][:].rearrange("p (b f) -> p b f", b=NB)[:, :, src0:src0 + n_el],
+                nc.vector.scalar_tensor_tensor(out=res[:].rearrange("p (b f) -> p b f", b=NB)[:, b0:b1, dst0:dst0 + n_el],
+                                               in0=negs[ob][:].rearrange("p (b f) -> p b f", b=NB)[:, b0:b1, src0:src0 + n_el],
                                                scalar=one_minus_a[:, 0:1],
-                                               in1=ns[ob][:].rearrange("p (b f) -> p b f", b=NB)[:, :, src0:src0 + n_el],
+                                               in1=ns[ob][:].rearrange("p (b f) -> p b f", b=NB)[:, b0:b1, src0:src0 + n_el],
                                                op0=ALU.mult, op1=ALU.add)
-            nc.sync.dma_start(out=out_v[:, ob], in_=res[:].rearrange("p (b f) -> p b f", b=NB))
+            nc.sync.dma_start(out=out_v[:, ob, b0:b1], in_=res[:].rearrange("p (b f) -> p b f", b=NB)[:, b0:b1])
 
         B6 = STEPS - 2
         B7 = STEPS - 1
@@ -773,6 +795,7 @@ def tile_merge_pa_kernel(tc, x, w_c1, b_c1, w_q, w_k, w_v, bn_gamma, bn_beta, pr
         divide_block(B7, 0)
         last_sum(0)
         last_squares(0)
+        moments(STEPS - 4, 6, 8)
         divide_block(B6, 1)
         divide_block(B7, 1)
         totals(0)
@@ -801,7 +824,8 @@ def tile_merge_pa_kernel(tc, x, w_c1, b_c1, w_q, w_k, w_v, bn_gamma, bn_beta, pr
         statistics(3)
         prelu_and_store(1)
         normalise(3)
-        minus_part(3, True)
+        last_parts()
         minus_part(2)
         prelu_and_store(2)
-        prelu_and_store(3)
+        prelu_and_store(3, 0, 2)
+        prelu_and_store(3, 2, 4)

@@ -31,6 +31,7 @@ PIECES = ((0, 4), (4, 4), (8, 8))
 HAAR_ON_VECTOR = ((0, 0), (0, 1), (1, 2), (1, 3), (2, 0), (2, 1), (2, 2))
 W_C1, W_K, W_Q, W_V, W_KN = 0, 1, 2, 3, 4
 CENTRE = 4
+FIRST_SLOTS = (1, 6, 0, 2, 3, 4, 5, 7)
 AROUND = (0, 1, 2, 3, 5, 6, 7, 8)
 OFFSET_OF_SLOT = AROUND + (CENTRE,)
 GROUPS = ((0, 3), (3, 6), (6, 8))
@@ -190,6 +191,12 @@ def tile_merge_pa_kernel(tc, x, w_c1, b_c1, w_q, w_k, w_v, bn_gamma, bn_beta, pr
                 q_ps = psm.tile([P, 512], F32, name="q_ps", tag="k_ps", bufs=3)
                 conv(q_ps[:], s, 4, W_Q)
                 banks[tok] = q_ps
+            elif kind == "K":
+                k_ps = psm.tile([P, 512], F32, name="k_ps", tag="k_ps", bufs=3)
+                conv(k_ps[:], s, AROUND[j], W_K, True, False)
+                banks[("k", s, j)] = k_ps
+            elif kind == "k" and ("K", s, j) in done:
+                conv(banks[tok][:], s, CENTRE, W_KN, False, True)
             elif kind == "k":
                 if j == AHEAD and s >= FIRST_LENT:
                     k_ps = psm.tile([P, 512], F32, name="k_lent", tag="den", bufs=1)
@@ -202,8 +209,10 @@ def tile_merge_pa_kernel(tc, x, w_c1, b_c1, w_q, w_k, w_v, bn_gamma, bn_beta, pr
                     window(k_ps[:], LAST_WINDOWS[j][0], LAST_WINDOWS[j][1], W_K, True, True)
                 banks[tok] = k_ps
             elif kind == "d":
-                idle = psm.tile([P, 512], F32, name="idle", tag="num", bufs=1)
-                nc.tensor.matmul_mx(out=idle[:], lhsT=w_codes[W_KN][:, 0:P].bitcast(FP8X4), lhsT_scale=w_scales[W_KN][:, 0:P],
+                if j == 0:
+                    idle = psm.tile([P, 512], F32, name="idle", tag="num", bufs=1)
+                    banks["idle"] = idle
+                nc.tensor.matmul_mx(out=banks["idle"][:], lhsT=w_codes[W_KN][:, 0:P].bitcast(FP8X4), lhsT_scale=w_scales[W_KN][:, 0:P],
                                     rhs=w_codes[W_KN][:].bitcast(FP8X4), rhs_scale=w_scales[W_KN][:], start=True, stop=True)
             elif kind in ("v", "u"):
                 if tok in in_k_banks:
@@ -311,6 +320,9 @@ def tile_merge_pa_kernel(tc, x, w_c1, b_c1, w_q, w_k, w_v, bn_gamma, bn_beta, pr
         def scores_of(s):
             return len(LAST_WINDOWS) if s == LAST else 8
 
+        def slot_of(s, i):
+            return FIRST_SLOTS[i] if s == 0 else i
+
         def den_terms(s):
             return 4 * len(LAST_EXPS) if s == LAST else 36
 
@@ -319,11 +331,11 @@ def tile_merge_pa_kernel(tc, x, w_c1, b_c1, w_q, w_k, w_v, bn_gamma, bn_beta, pr
 
         pe_list = [("d", 0, i) for i in range(WARM_UP)] + [("w", W_C1, 0), ("w", W_C1, 1)] + on_pe(0) + [("w", W_Q, 0), ("w", W_Q, 1), ("c", 0, 0), ("c", 1, 0),
                                                                  ("w", W_K, 0), ("w", W_K, 1)] + on_pe(1)
-        pe_list += [("q", 0, 0)] + [("k", 0, j) for j in range(AHEAD)]
+        pe_list += [("q", 0, 0)] + [("K", 0, j) for j in FIRST_SLOTS[0:2]] + [("k", 0, j) for j in FIRST_SLOTS[0:AHEAD]]
         for s in range(STEPS + 2):
             a = s - 2
             if ok(s):
-                pe_list.extend([("k", s, j) for j in range(AHEAD if s == 0 else AHEAD + LATE, scores_of(s))])
+                pe_list.extend([("k", s, slot_of(s, j)) for j in range(AHEAD if s == 0 else AHEAD + LATE, scores_of(s))])
             if ok(s + 1) and s not in LATE_Q:
                 pe_list.append(("q", s + 1, 0))
             if s == 0:
@@ -399,7 +411,7 @@ def tile_merge_pa_kernel(tc, x, w_c1, b_c1, w_q, w_k, w_v, bn_gamma, bn_beta, pr
                 pump_to(tok)
                 halve(pc, tok[2], banks[tok][:, 0:ROW * PIECES[pc][1]])
 
-        def haar_on_vector(pc, images, on_gpsimd=False):
+        def haar_on_vector(pc, images, on_gpsimd=False, between=None):
             eng = nc.gpsimd if on_gpsimd else nc.vector
             nr = PIECES[pc][1]
             row_sums = []
@@ -411,11 +423,17 @@ def tile_merge_pa_kernel(tc, x, w_c1, b_c1, w_q, w_k, w_v, bn_gamma, bn_beta, pr
                     s1 = main.tile([P, 4, nr, 32], F32, name="s1", tag="s1", bufs=2)
                 eng.tensor_tensor(out=s1[:], in0=rows[:, :, :, 0, :], in1=rows[:, :, :, 1, :], op=ALU.add)
                 row_sums.append(s1)
+            sums = []
             for b, s1 in zip(images, row_sums):
                 pairs = s1[:].rearrange("p j i (x e) -> p (j i x) e", e=2)
                 s2 = main.tile([P, ROW * nr], F32, name="s2", tag="s2", bufs=3)
+                if between is not None and b == images[-1]:
+                    between()
                 eng.tensor_tensor(out=s2[:], in0=pairs[:, :, 0], in1=pairs[:, :, 1], op=ALU.add)
-                halve(pc, b, s2[:])
+                if between is None:
+                    halve(pc, b, s2[:])
+                sums.append((b, s2))
+            return sums
 
         def haar_by_reduce(pc, b):
             nr = PIECES[pc][1]
@@ -480,9 +498,10 @@ def tile_merge_pa_kernel(tc, x, w_c1, b_c1, w_q, w_k, w_v, bn_gamma, bn_beta, pr
             q_sbs[s] = q_sb
 
         def scores(s, j0, j1):
-            for j in range(j0, j1):
+            for i in range(j0, j1):
+                j = slot_of(s, i)
                 pump_to(("k", s, j))
-                if j == 0:
+                if i == 0:
                     z = main.tile([P, 9, 512], F32, name="z", tag="z", bufs=3)
                     zs[s] = z
                 nc.vector.tensor_tensor(out=zs[s][:, j, :], in0=q_sbs[s][:], in1=banks[("k", s, j)][:], op=ALU.mult)
@@ -604,17 +623,13 @@ def tile_merge_pa_kernel(tc, x, w_c1, b_c1, w_q, w_k, w_v, bn_gamma, bn_beta, pr
         g_k = weight_copies(W_K)
         quant_y(0)
         g_kn = main.tile([P, 2048], BF16, name="grouped_neg", tag="grouped", bufs=2, align_bytes=64)
-        def negate_half(h):
-            nc.vector.tensor_scalar(out=g_kn[:, 1024 * h:1024 * (h + 1)], in0=g_k[:, 1024 * h:1024 * (h + 1)], scalar1=-1.0, scalar2=None,
-                                    op0=ALU.mult)
-
-        negate_half(0)
+        nc.vector.tensor_scalar(out=g_kn[:, 0:1024], in0=g_k[:, 0:1024], scalar1=-1.0, scalar2=None, op0=ALU.mult)
+        nc.scalar.activation(out=g_kn[:, 1024:2048], in_=g_k[:, 1024:2048], func=ACT.Copy, scale=-1.0)
         quant_w_half(W_K, g_k, 0)
         quant_w_half(W_KN, g_kn, 0)
-        move_y(0)
-        negate_half(1)
         quant_w_half(W_K, g_k, 1)
         quant_w_half(W_KN, g_kn, 1)
+        move_y(0)
         q_copy(0)
         haar_from_pe(1)
 
@@ -623,6 +638,7 @@ def tile_merge_pa_kernel(tc, x, w_c1, b_c1, w_q, w_k, w_v, bn_gamma, bn_beta, pr
 
 
         haar_on_vector(1, (2, 3), True)
+        waiting = []
         scores(0, 0, AHEAD)
         for s in range(STEPS):
             scores(s, AHEAD, scores_of(s))
@@ -642,7 +658,7 @@ def tile_merge_pa_kernel(tc, x, w_c1, b_c1, w_q, w_k, w_v, bn_gamma, bn_beta, pr
                 quant_y(2)
             if s == 0:
                 shift_by_max(s, (lambda: (quant_ll(1), add_bias_on_scalar(1)()),
-                                 lambda: haar_on_vector(2, (0, 1)), lambda: quant_y(1)), 0, True)
+                                 lambda: waiting.extend(haar_on_vector(2, (0, 1), between=lambda: quant_y(1))), nothing), 0, True)
             elif s == 1:
                 shift_by_max(s, (lambda: quant_ll(2), lambda: quant_w(W_V, g_v), nothing), 0, True)
                 scores(s + 1, 0, AHEAD)
@@ -656,6 +672,8 @@ def tile_merge_pa_kernel(tc, x, w_c1, b_c1, w_q, w_k, w_v, bn_gamma, bn_beta, pr
                     scores(s + 1, 0, AHEAD)
             if s == 0:
                 q_copy(1)
+                for b, s2 in waiting:
+                    halve(2, b, s2[:])
                 move_y(1)
                 g_v = weight_copies(W_V)
                 haar_from_pe(2)

@@ -314,8 +314,8 @@ def tile_merge_pa_kernel(tc, x, w_c1, b_c1, w_q, w_k, w_v, bn_gamma, bn_beta, pr
                     toks.append(tok)
             return toks
 
-        lent_to_v = [v_banks(a)[3] for a in range(STEPS - 2)]
-        in_k_banks = v_banks(STEPS - 2)[3:] + v_banks(STEPS - 1)[3:]
+        lent_to_v = [v_banks(a)[3] for a in range(STEPS - 3)]
+        in_k_banks = v_banks(STEPS - 3)[3:] + v_banks(STEPS - 2)[3:] + v_banks(STEPS - 1)[3:]
 
         def scores_of(s):
             return len(LAST_WINDOWS) if s == LAST else 8
@@ -354,7 +354,7 @@ def tile_merge_pa_kernel(tc, x, w_c1, b_c1, w_q, w_k, w_v, bn_gamma, bn_beta, pr
                 pe_list.extend(vb)
                 vb = []
             if s == STEPS - 1:
-                pe_list.extend(den_sums + vb)
+                pe_list.extend(vb + den_sums)
                 vb = []
                 den_sums = []
             if ok(a) and a < EARLY_FROM:
@@ -822,23 +822,23 @@ def tile_merge_pa_kernel(tc, x, w_c1, b_c1, w_q, w_k, w_v, bn_gamma, bn_beta, pr
         last_squares(1)
         normalise(0)
         divide_block(B6, 2)
-        divide_block(B7, 2)
         totals(1)
+        divide_block(B7, 2)
         statistics(1)
         last_sum(2)
         last_squares(2)
         normalise(1)
         minus_part(0)
         divide_block(B6, 3)
-        divide_block(B7, 3)
         totals(2)
+        divide_block(B7, 3)
         statistics(2)
         last_sum(3)
         last_squares(3)
         prelu_and_store(0)
         normalise(2)
-        minus_part(1)
         totals(3)
+        minus_part(1)
         statistics(3)
         prelu_and_store(1)
         normalise(3)

@@ -285,7 +285,7 @@ def tile_merge_pa_kernel(tc, x, w_c1, b_c1, w_q, w_k, w_v, bn_gamma, bn_beta, pr
                 if j % 6 == 0:
                     last_bank(s, ob)
                 nc.tensor.matmul(out=nums[(s, ob)][:], lhsT=evs[s][:, j % 6, P * ob:P * (ob + 1)], rhs=to_ybx[:],
-                                 is_transpose=True, start=(j % 6 == 0), stop=(j % 6 == 5))
+                                 is_transpose=True, start=(j % 6 == 0), stop=(j % 6 == (2 if ob < 1 else 5)))
             else:
                 if j == 0:
                     num = psm.tile([P, 4, P], F32, name="num", tag="num", bufs=1)
@@ -373,7 +373,7 @@ def tile_merge_pa_kernel(tc, x, w_c1, b_c1, w_q, w_k, w_v, bn_gamma, bn_beta, pr
                 pe_list.extend([("k", s + 1, AHEAD + j) for j in range(LATE)])
         for ob in range(4):
             pe_list.extend([("G", STEPS - 2, 6 * ob + j) for j in range(6)])
-            pe_list.extend([("G", STEPS - 1, 6 * ob + j) for j in range(6)])
+            pe_list.extend([("G", STEPS - 1, 6 * ob + j) for j in range(3 if ob < 1 else 6)])
 
         done = set()
         pos = [0]
@@ -716,6 +716,8 @@ def tile_merge_pa_kernel(tc, x, w_c1, b_c1, w_q, w_k, w_v, bn_gamma, bn_beta, pr
         exps(STEPS - 1, 1)
         root_of_last_den(STEPS - 2)
         weigh(STEPS - 1, 0, 6)
+        ev7 = evs[STEPS - 1]
+        nc.vector.tensor_tensor(out=ev7[:, 0:3, 0:128], in0=ev7[:, 0:3, 0:128], in1=ev7[:, 3:6, 0:128], op=ALU.add)
         root_of_last_den(STEPS - 1)
         moments(STEPS - 4, 3, 6)
 
@@ -737,7 +739,7 @@ def tile_merge_pa_kernel(tc, x, w_c1, b_c1, w_q, w_k, w_v, bn_gamma, bn_beta, pr
         part = {}
 
         def divide_block(s, ob):
-            pump_to(("G", s, 6 * ob + 5))
+            pump_to(("G", s, 6 * ob + (2 if s == STEPS - 1 and ob < 1 else 5)))
             if ob not in part:
                 once = main.tile([P, 2, P], F32, name="once", tag="once")
                 part[ob] = once

@@ -416,13 +416,15 @@ def tile_merge_pa_kernel(tc, x, w_c1, b_c1, w_q, w_k, w_v, bn_gamma, bn_beta, pr
             nr = PIECES[pc][1]
             row_sums = []
             for b in images:
-                rows = x_piece(pc, b).rearrange("p j (i a w) -> p j i a w", a=2, w=32)
                 if on_gpsimd:
                     s1 = main.tile([P, 4, nr, 32], F32, name="s1_late", tag="grouped", bufs=2, align_bytes=64)
+                    row_sums.insert(0, s1)
                 else:
                     s1 = main.tile([P, 4, nr, 32], F32, name="s1", tag="s1", bufs=2)
+                    row_sums.append(s1)
+            for b, s1 in zip(images, row_sums):
+                rows = x_piece(pc, b).rearrange("p j (i a w) -> p j i a w", a=2, w=32)
                 eng.tensor_tensor(out=s1[:], in0=rows[:, :, :, 0, :], in1=rows[:, :, :, 1, :], op=ALU.add)
-                row_sums.append(s1)
             sums = []
             for b, s1 in zip(images, row_sums):
                 pairs = s1[:].rearrange("p j i (x e) -> p (j i x) e", e=2)
@@ -628,8 +630,8 @@ def tile_merge_pa_kernel(tc, x, w_c1, b_c1, w_q, w_k, w_v, bn_gamma, bn_beta, pr
         quant_w_half(W_K, g_k, 0)
         quant_w_half(W_KN, g_kn, 0)
         quant_w_half(W_K, g_k, 1)
-        quant_w_half(W_KN, g_kn, 1)
         move_y(0)
+        quant_w_half(W_KN, g_kn, 1)
         q_copy(0)
         haar_from_pe(1)
 

@@ -418,7 +418,7 @@ def tile_merge_pa_kernel(tc, x, w_c1, b_c1, w_q, w_k, w_v, bn_gamma, bn_beta, pr
             for b in images:
                 if on_gpsimd:
                     s1 = main.tile([P, 4, nr, 32], F32, name="s1_late", tag="grouped", bufs=2, align_bytes=64)
-                    row_sums.insert(0, s1)
+                    row_sums.append(s1)
                 else:
                     s1 = main.tile([P, 4, nr, 32], F32, name="s1", tag="s1", bufs=2)
                     row_sums.append(s1)
@@ -639,6 +639,8 @@ def tile_merge_pa_kernel(tc, x, w_c1, b_c1, w_q, w_k, w_v, bn_gamma, bn_beta, pr
             return None
 
 
+        after_head = keep.tile([P, 1], I32, name="after_head")
+        nc.gpsimd.tensor_copy(out=after_head[:], in_=w_codes[W_KN][:, 511:512])
         haar_on_vector(1, (2, 3), True)
         waiting = []
         scores(0, 0, AHEAD)

@@ -28,7 +28,8 @@ LATE = 2
 LAST_BANKS = (("k_ps", 3), ("k_ps", 3), ("k_ps", 3), ("v_ps", 3), ("v_ps", 3), ("v_ps", 3), ("den", 1), ("num", 1))
 LAST_ON_VECTOR = 3
 PIECES = ((0, 4), (4, 4), (8, 8))
-HAAR_ON_VECTOR = ((0, 0), (0, 1), (1, 2), (1, 3), (2, 0), (2, 1), (2, 2))
+HAAR_ON_VECTOR = ((0, 0), (0, 1), (1, 2), (1, 3), (2, 2))
+TURNED = (0, 1)
 W_C1, W_K, W_Q, W_V, W_KN = 0, 1, 2, 3, 4
 CENTRE = 4
 FIRST_SLOTS = (1, 6, 0, 2, 3, 4, 5, 7)
@@ -141,6 +142,12 @@ def tile_merge_pa_kernel(tc, x, w_c1, b_c1, w_q, w_k, w_v, bn_gamma, bn_beta, pr
         nc.sync.dma_start(out=bet_bf[:], in_=bn_beta.rearrange("(p t) -> p t", t=4))
         nc.sync.dma_start(out=a_bf[:], in_=prelu_a.partition_broadcast(P))
 
+        haar_sum = keep.tile([P, 32], BF16, name="haar_sum")
+        with nc.allow_low_precision(reason="every sum is a single one"):
+            nc.vector.tensor_reduce(out=haar_sum[:].rearrange("p (i x) -> p i x", i=2),
+                                    in_=ident_bf[:].rearrange("p (i a x e) -> p i x a e", i=2, a=2, x=16), axis=mybir.AxisListType.XY,
+                                    op=ALU.add)
+        x_turned = {}
         zs = {}
         evs = {}
         nums = {}
@@ -256,9 +263,23 @@ def tile_merge_pa_kernel(tc, x, w_c1, b_c1, w_q, w_k, w_v, bn_gamma, bn_beta, pr
                     hs = psm.tile([P, 512], F32, name="hs_last", tag="den", bufs=1)
                 else:
                     hs = psm.tile([P, 512], F32, name="hs", tag="v_ps", bufs=3)
+                nj = 2 if s == 2 else 4
                 for n in range(4):
-                    nc.tensor.matmul(out=hs[:, 0:ROW * nr].rearrange("p (j i x) -> p j i x", j=4, x=16), lhsT=ident_bf[:],
-                                     rhs=taps[:, :, :, n // 2, :, n % 2], start=(n == 0), stop=(n == 3))
+                    nc.tensor.matmul(out=hs[:, 0:16 * nj * nr].rearrange("p (j i x) -> p j i x", j=nj, x=16), lhsT=ident_bf[:],
+                                     rhs=taps[:, 0:nj, :, n // 2, :, n % 2], start=(n == 0), stop=(n == 3))
+                banks[tok] = hs
+            elif kind == "T":
+                xt = psm.tile([P, 8, P], BF16, name="xt", tag="v_ps", bufs=3)
+                for i in range(8):
+                    nc.tensor.transpose(xt[:, i, :], x_c[:, s, 2 * j + i // 4, P * (i % 4):P * (i % 4 + 1)], ident_bf[:])
+                banks[tok] = xt
+            elif kind == "H":
+                if s == NB - 1:
+                    hs = banks[("h", 2, s)]
+                else:
+                    hs = psm.tile([P, 512], F32, name="hs_turned", tag="v_ps", bufs=3)
+                for i in range(8 if s == NB - 1 else 0, 16):
+                    nc.tensor.matmul(out=hs[:, 32 * i:32 * (i + 1)], lhsT=x_turned[s][:, i, :], rhs=haar_sum[:], start=True, stop=True)
                 banks[tok] = hs
             elif kind == "F":
                 if j == 0:
@@ -327,7 +348,7 @@ def tile_merge_pa_kernel(tc, x, w_c1, b_c1, w_q, w_k, w_v, bn_gamma, bn_beta, pr
             return 4 * len(LAST_EXPS) if s == LAST else 36
 
         def on_pe(pc):
-            return [("h", pc, b) for b in range(NB) if (pc, b) not in HAAR_ON_VECTOR]
+            return [("h", pc, b) for b in range(NB) if (pc, b) not in HAAR_ON_VECTOR and (pc < 2 or b not in TURNED)]
 
         pe_list = [("d", 0, i) for i in range(WARM_UP)] + [("w", W_C1, 0), ("w", W_C1, 1)] + on_pe(0) + [("w", W_Q, 0), ("w", W_Q, 1), ("c", 0, 0), ("c", 1, 0),
                                                                  ("w", W_K, 0), ("w", W_K, 1)] + on_pe(1)
@@ -339,9 +360,10 @@ def tile_merge_pa_kernel(tc, x, w_c1, b_c1, w_q, w_k, w_v, bn_gamma, bn_beta, pr
             if ok(s + 1) and s not in LATE_Q:
                 pe_list.append(("q", s + 1, 0))
             if s == 0:
-                pe_list.extend([("C", 1, t) for t in range(4)] + [("w", W_V, 0), ("w", W_V, 1)] + on_pe(2))
+                pe_list.extend([("C", 1, t) for t in range(4)] + [("T", 0, 0), ("T", 0, 1), ("T", 1, 0)] + on_pe(2))
             if s == 1:
-                pe_list.extend([("C", 2, t) for t in range(4)])
+                pe_list.extend([("T", 1, 1), ("H", 0, 0), ("T", 3, 1), ("H", 1, 0), ("H", 3, 0), ("w", W_V, 0), ("w", W_V, 1)])
+                pe_list.extend([("k", s + 1, j) for j in range(AHEAD)] + [("C", 2, t) for t in range(4)])
             vb = v_banks(a)[3 if a >= EARLY_FROM else 0:] if ok(a) else []
             early = v_banks(a + 1)[:3] if ok(a + 1) and a + 1 >= EARLY_FROM else []
             den_sums = [("F", a, i) for i in range(den_terms(a))] if ok(a) else []
@@ -364,7 +386,7 @@ def tile_merge_pa_kernel(tc, x, w_c1, b_c1, w_q, w_k, w_v, bn_gamma, bn_beta, pr
             if s in LATE_Q:
                 pe_list.extend(den_sums[18:] + [("q", s + 1, 0)])
                 den_sums = den_sums[:18]
-            if ok(s + 1):
+            if ok(s + 1) and s != 1:
                 pe_list.extend([("k", s + 1, j) for j in range(AHEAD)])
             pe_list.extend(den_sums[18:])
             pe_list.extend(num_sums)
@@ -443,6 +465,19 @@ def tile_merge_pa_kernel(tc, x, w_c1, b_c1, w_q, w_k, w_v, bn_gamma, bn_beta, pr
             s2 = main.tile([P, ROW * nr], F32, name="s2_red", tag="s2", bufs=3)
             nc.vector.tensor_reduce(out=s2[:].rearrange("p (j i x) -> p j i x", j=4, x=16), in_=taps, axis=mybir.AxisListType.XY, op=ALU.add)
             return s2
+
+        def turn_copies(b, halves):
+            if b not in x_turned:
+                turned = main.tile([P, 16, P], BF16, name="turned", tag="s1", bufs=2)
+                x_turned[b] = turned
+            for h in halves:
+                pump_to(("T", b, h))
+                nc.scalar.copy(out=x_turned[b][:, 8 * h:8 * (h + 1)].rearrange("p i c -> p (i c)").bitcast(F32),
+                               in_=banks[("T", b, h)][:].rearrange("p i c -> p (i c)").bitcast(F32))
+
+        def haar_from_turned(b):
+            pump_to(("H", b, 0))
+            halve(2, b, banks[("H", b, 0)][:])
 
         def quant_ll(pc):
             c0 = ROW * PIECES[pc][0]
@@ -612,6 +647,9 @@ def tile_merge_pa_kernel(tc, x, w_c1, b_c1, w_q, w_k, w_v, bn_gamma, bn_beta, pr
                                      bias=neg_pivot[:, ob:ob + 1], scale=1.0,
                                      accum_out=msums[:, kind, ob, s // 2:s // 2 + 1])
 
+        def nothing():
+            return None
+
         g_c1 = weight_copies(W_C1)
         haar_on_vector(0, (0, 1))
         quant_w(W_C1, g_c1)
@@ -635,14 +673,10 @@ def tile_merge_pa_kernel(tc, x, w_c1, b_c1, w_q, w_k, w_v, bn_gamma, bn_beta, pr
         q_copy(0)
         haar_from_pe(1)
 
-        def nothing():
-            return None
-
 
         after_head = keep.tile([P, 1], I32, name="after_head")
         nc.gpsimd.tensor_copy(out=after_head[:], in_=w_codes[W_KN][:, 511:512])
         haar_on_vector(1, (2, 3), True)
-        waiting = []
         scores(0, 0, AHEAD)
         for s in range(STEPS):
             scores(s, AHEAD, scores_of(s))
@@ -655,14 +689,21 @@ def tile_merge_pa_kernel(tc, x, w_c1, b_c1, w_q, w_k, w_v, bn_gamma, bn_beta, pr
             if ok(s + 1) and s not in LATE_Q:
                 q_copy(s + 1)
             if s == 1:
+                turn_copies(1, (1,))
+                haar_from_turned(0)
+                turn_copies(3, (1,))
+                haar_from_turned(1)
                 halve(2, 2, late_sums[:])
+                haar_from_turned(3)
+                g_v = weight_copies(W_V)
             if ok(s - 2):
                 weigh(s - 2, 0, 12)
             if s == 2:
                 quant_y(2)
             if s == 0:
-                shift_by_max(s, (lambda: (quant_ll(1), add_bias_on_scalar(1)()),
-                                 lambda: waiting.extend(haar_on_vector(2, (0, 1), between=lambda: quant_y(1))), nothing), 0, True)
+                quant_ll(1)
+                add_bias_on_scalar(1)()
+                shift_by_max(s, (nothing, lambda: quant_y(1), nothing), 0, True)
             elif s == 1:
                 shift_by_max(s, (lambda: quant_ll(2), lambda: quant_w(W_V, g_v), nothing), 0, True)
                 scores(s + 1, 0, AHEAD)
@@ -676,17 +717,14 @@ def tile_merge_pa_kernel(tc, x, w_c1, b_c1, w_q, w_k, w_v, bn_gamma, bn_beta, pr
                     scores(s + 1, 0, AHEAD)
             if s == 0:
                 q_copy(1)
-                for b, s2 in waiting:
-                    halve(2, b, s2[:])
+                turn_copies(0, (0, 1))
+                turn_copies(1, (0,))
                 move_y(1)
-                g_v = weight_copies(W_V)
-                haar_from_pe(2)
                 scores(1, 0, AHEAD)
             if s == 1:
-                weave = add_bias_on_scalar(2)
                 exps(0, 1)
-                weave()
                 exps(0, 2)
+                add_bias_on_scalar(2)()
             elif ok(s - 1) and s != 2:
                 if s == STEPS - 1:
                     one_over_den(s - 2)

@@ -376,7 +376,7 @@ def tile_merge_pa_kernel(tc, x, w_c1, b_c1, w_q, w_k, w_v, bn_gamma, bn_beta, pr
                 pe_list.extend(vb)
                 vb = []
             if s == STEPS - 1:
-                pe_list.extend(vb + den_sums)
+                pe_list.extend(den_sums[:9] + vb + den_sums[9:])
                 vb = []
                 den_sums = []
             if ok(a) and a < EARLY_FROM:
@@ -422,10 +422,10 @@ def tile_merge_pa_kernel(tc, x, w_c1, b_c1, w_q, w_k, w_v, bn_gamma, bn_beta, pr
             nc.vector.quantize_mx(out=w_codes[i][:, 256 * h:256 * (h + 1)].bitcast(FP8X4), scales=w_scales[i][:, 256 * h:256 * (h + 1)],
                                   in_=grouped[:, 1024 * h:1024 * (h + 1)])
 
-        def halve(pc, b, sums):
+        def halve(pc, b, sums, j0=0, j1=4):
             row0, nr = PIECES[pc]
-            nc.scalar.activation(out=ll_by_image[:, b, row0:row0 + nr],
-                                 in_=sums.rearrange("p (j y x) -> p y x j", j=4, x=16),
+            nc.scalar.activation(out=ll_by_image[:, b, row0:row0 + nr, :, j0:j1],
+                                 in_=sums.rearrange("p (j y x) -> p y x j", j=j1 - j0, x=16),
                                  func=ACT.Copy, scale=0.5)
 
         def haar_from_pe(pc):
@@ -475,9 +475,9 @@ def tile_merge_pa_kernel(tc, x, w_c1, b_c1, w_q, w_k, w_v, bn_gamma, bn_beta, pr
                 nc.scalar.copy(out=x_turned[b][:, 8 * h:8 * (h + 1)].rearrange("p i c -> p (i c)").bitcast(F32),
                                in_=banks[("T", b, h)][:].rearrange("p i c -> p (i c)").bitcast(F32))
 
-        def haar_from_turned(b):
+        def haar_from_turned(b, j0=0):
             pump_to(("H", b, 0))
-            halve(2, b, banks[("H", b, 0)][:])
+            halve(2, b, banks[("H", b, 0)][:, P * j0:512], j0)
 
         def quant_ll(pc):
             c0 = ROW * PIECES[pc][0]
@@ -549,7 +549,7 @@ def tile_merge_pa_kernel(tc, x, w_c1, b_c1, w_q, w_k, w_v, bn_gamma, bn_beta, pr
             eng.tensor_tensor(out=z[:, g0:g1, :], in0=z[:, g0:g1, :], in1=ms[s][:].unsqueeze(1).to_broadcast([P, g1 - g0, 512]),
                               op=ALU.subtract)
 
-        def tree_in_halves(s, between, on_vector=0):
+        def tree_in_halves(s, between, on_vector=0, before_m=None):
             z = zs[s]
             halves = (slice(0, 256), slice(256, 512))
             n = scores_of(s) // 2
@@ -560,6 +560,8 @@ def tile_merge_pa_kernel(tc, x, w_c1, b_c1, w_q, w_k, w_v, bn_gamma, bn_beta, pr
             t2 = main.tile([P, 2, 512], F32, name="t2", tag="t2", bufs=1)
             for c in halves:
                 nc.vector.tensor_tensor(out=t2[:, 0:n // 2, c], in0=t1[:, 0:n // 2, c], in1=t1[:, n // 2:2 * (n // 2), c], op=ALU.max)
+            if before_m is not None:
+                before_m()
             m = main.tile([P, 512], F32, name="m", tag="m")
             for c in halves:
                 other = t1[:, 2, c] if s == LAST else t2[:, 1, c]
@@ -676,6 +678,12 @@ def tile_merge_pa_kernel(tc, x, w_c1, b_c1, w_q, w_k, w_v, bn_gamma, bn_beta, pr
 
         after_head = keep.tile([P, 1], I32, name="after_head")
         nc.gpsimd.tensor_copy(out=after_head[:], in_=w_codes[W_KN][:, 511:512])
+        def in_waits(s, part):
+            if s in (4, 5):
+                moments(0, 4 * (s - 4) + 2 * part, 4 * (s - 4) + 2 * part + 2)
+            elif s == 6:
+                moments(2, 2 * part, 2 * part + 2)
+
         haar_on_vector(1, (2, 3), True)
         scores(0, 0, AHEAD)
         for s in range(STEPS):
@@ -694,7 +702,7 @@ def tile_merge_pa_kernel(tc, x, w_c1, b_c1, w_q, w_k, w_v, bn_gamma, bn_beta, pr
                 turn_copies(3, (1,))
                 haar_from_turned(1)
                 halve(2, 2, late_sums[:])
-                haar_from_turned(3)
+                haar_from_turned(3, 2)
                 g_v = weight_copies(W_V)
             if ok(s - 2):
                 weigh(s - 2, 0, 12)
@@ -703,7 +711,7 @@ def tile_merge_pa_kernel(tc, x, w_c1, b_c1, w_q, w_k, w_v, bn_gamma, bn_beta, pr
             if s == 0:
                 quant_ll(1)
                 add_bias_on_scalar(1)()
-                shift_by_max(s, (nothing, lambda: quant_y(1), nothing), 0, True)
+                tree_in_halves(s, nothing, 0, lambda: quant_y(1))
             elif s == 1:
                 shift_by_max(s, (lambda: quant_ll(2), lambda: quant_w(W_V, g_v), nothing), 0, True)
                 scores(s + 1, 0, AHEAD)
@@ -719,6 +727,8 @@ def tile_merge_pa_kernel(tc, x, w_c1, b_c1, w_q, w_k, w_v, bn_gamma, bn_beta, pr
                 q_copy(1)
                 turn_copies(0, (0, 1))
                 turn_copies(1, (0,))
+                pump_to(("h", 2, 3))
+                halve(2, 3, banks[("h", 2, 3)][:, 0:256], 0, 2)
                 move_y(1)
                 scores(1, 0, AHEAD)
             if s == 1:
@@ -728,7 +738,12 @@ def tile_merge_pa_kernel(tc, x, w_c1, b_c1, w_q, w_k, w_v, bn_gamma, bn_beta, pr
             elif ok(s - 1) and s != 2:
                 if s == STEPS - 1:
                     one_over_den(s - 2)
+                in_waits(s, 0)
                 exps(s - 1, 1)
+                in_waits(s, 1)
+                if s == STEPS - 1:
+                    neg_m = main.tile([P, 512], F32, name="neg_m", tag="m")
+                    nc.scalar.activation(out=neg_m[:], in_=ms[s][:], func=ACT.Copy, scale=-1.0)
                 exps(s - 1, 2)
             if ok(s - 2) and s < STEPS - 1:
                 one_over_den(s - 2)
@@ -737,11 +752,9 @@ def tile_merge_pa_kernel(tc, x, w_c1, b_c1, w_q, w_k, w_v, bn_gamma, bn_beta, pr
                 nc.scalar.activation(out=msums[:, 0, :, PAIRS], in_=att[:, :, 0], func=ACT.Copy, scale=-2.0 * P)
                 nc.scalar.activation(out=one_minus_a[:], in_=a_bf[:], func=ACT.Identity, bias=1.0, scale=-1.0)
                 nc.scalar.copy(out=gam_f[:], in_=gam_bf[:])
-            if ok(s - 3) and (s - 3) % 2 == 1:
-                moments(s - 4)
+            if s == 6:
+                moments(2, 4, 8)
         lg_end = keep.tile([P, 4, 2, P], F32, name="lg_end")
-        neg_m = main.tile([P, 512], F32, name="neg_m", tag="m")
-        nc.scalar.activation(out=neg_m[:], in_=ms[STEPS - 1][:], func=ACT.Copy, scale=-1.0)
         z_last = zs[STEPS - 1]
         for g0, g1 in GROUPS[1:2]:
             nc.gpsimd.tensor_tensor(out=z_last[:, g0:g1, :], in0=z_last[:, g0:g1, :],
@@ -872,8 +885,8 @@ def tile_merge_pa_kernel(tc, x, w_c1, b_c1, w_q, w_k, w_v, bn_gamma, bn_beta, pr
         last_sum(2)
         last_squares(2)
         normalise(1)
-        minus_part(0)
         divide_block(B6, 3)
+        minus_part(0)
         totals(2)
         divide_block(B7, 3)
         statistics(2)

@@ -57,9 +57,9 @@ def tile_merge_pa_kernel(tc, x, w_c1, b_c1, w_q, w_k, w_v, bn_gamma, bn_beta, pr
         ctx.enter_context(tc.manual_schedule())
 
         weights = (w_c1, w_k, w_q, w_v)
-        w_all = main.tile([P, 4, 4, 512], BF16, name="w_all", tag="z", bufs=3)
-        x_ab = main.tile([P, 2, NB, 4, 256], BF16, name="x_ab", tag="ev", bufs=2)
-        x_c = main.tile([P, NB, 4, 512], BF16, name="x_c", tag="ev", bufs=2)
+        w_all = main.tile([P, 4, 4, 512], BF16, name="w_all", tag="z", bufs=3, align_bytes=256)
+        x_ab = main.tile([P, 2, NB, 4, 256], BF16, name="x_ab", tag="ev", bufs=2, align_bytes=256)
+        x_c = main.tile([P, NB, 4, 512], BF16, name="x_c", tag="ev", bufs=2, align_bytes=256)
 
         def x_piece(pc, b):
             return x_c[:, b] if pc == 2 else x_ab[:, pc, b]
@@ -80,17 +80,17 @@ def tile_merge_pa_kernel(tc, x, w_c1, b_c1, w_q, w_k, w_v, bn_gamma, bn_beta, pr
         load_w(W_C1)
         load_x(0)
         nc.sync.dma_start(out=bias_bf[:], in_=b_c1.rearrange("(p t) -> p t", t=4))
-        load_w(W_Q)
+        load_w(W_Q, 2)
         load_w(W_K, 2)
         load_x(1)
         load_w(W_V)
         load_x(2)
 
-        ident = keep.tile([P, P], F32, name="ident")
+        ident = keep.tile([P, P], F32, name="ident", align_bytes=256)
         make_identity(nc, ident[:])
         ident_bf = keep.tile([P, P], BF16, name="ident_bf")
         make_identity(nc, ident_bf[:])
-        to_ybx = keep.tile([P, P], F32, name="to_ybx")
+        to_ybx = keep.tile([P, P], F32, name="to_ybx", align_bytes=256)
         nc.gpsimd.tensor_copy(out=to_ybx[:].rearrange("p (y b x) -> p y b x", b=NB, x=16),
                               in_=ident[:].rearrange("p (y x b) -> p y b x", b=NB, x=16))
 
@@ -104,8 +104,8 @@ def tile_merge_pa_kernel(tc, x, w_c1, b_c1, w_q, w_k, w_v, bn_gamma, bn_beta, pr
         w_codes = []
         w_scales = []
         for i in range(5):
-            wct = keep.tile([P, 512], I32, name="w_codes%d" % i, align_bytes=64)
-            wst = keep.tile([P, 512], U8, name="w_scales%d" % i, align_bytes=64)
+            wct = keep.tile([P, 512], I32, name="w_codes%d" % i, align_bytes=256)
+            wst = keep.tile([P, 512], U8, name="w_scales%d" % i, align_bytes=256)
             w_codes.append(wct)
             w_scales.append(wst)
         nc.vector.memset(w_codes[W_KN][:], 0)
@@ -115,8 +115,8 @@ def tile_merge_pa_kernel(tc, x, w_c1, b_c1, w_q, w_k, w_v, bn_gamma, bn_beta, pr
         y_codes = []
         y_scales = []
         for d in range(3):
-            yct = keep.tile([P, Y_ROWS * ROW], I32, name="y_codes%d" % d, align_bytes=64)
-            yst = keep.tile([P, Y_ROWS * ROW], U8, name="y_scales%d" % d, align_bytes=64)
+            yct = keep.tile([P, Y_ROWS * ROW], I32, name="y_codes%d" % d, align_bytes=256)
+            yst = keep.tile([P, Y_ROWS * ROW], U8, name="y_scales%d" % d, align_bytes=256)
             if d != 1:
                 nc.gpsimd.memset(yct[:].bitcast(F32), 0.0)
             nc.gpsimd.memset(yst[:].bitcast(F32), 0.0)
@@ -360,9 +360,9 @@ def tile_merge_pa_kernel(tc, x, w_c1, b_c1, w_q, w_k, w_v, bn_gamma, bn_beta, pr
             if ok(s + 1) and s not in LATE_Q:
                 pe_list.append(("q", s + 1, 0))
             if s == 0:
-                pe_list.extend([("C", 1, t) for t in range(4)] + [("T", 0, 0), ("T", 0, 1), ("T", 1, 0)] + on_pe(2))
+                pe_list.extend([("w", W_V, 0), ("w", W_V, 1)] + [("C", 1, t) for t in range(4)] + [("T", 0, 0), ("T", 0, 1), ("T", 1, 0)] + on_pe(2))
             if s == 1:
-                pe_list.extend([("T", 1, 1), ("H", 0, 0), ("T", 3, 1), ("H", 1, 0), ("H", 3, 0), ("w", W_V, 0), ("w", W_V, 1)])
+                pe_list.extend([("T", 1, 1), ("H", 0, 0), ("T", 3, 1), ("H", 1, 0), ("H", 3, 0)])
                 pe_list.extend([("k", s + 1, j) for j in range(AHEAD)] + [("C", 2, t) for t in range(4)])
             vb = v_banks(a)[3 if a >= EARLY_FROM else 0:] if ok(a) else []
             early = v_banks(a + 1)[:3] if ok(a + 1) and a + 1 >= EARLY_FROM else []
@@ -539,7 +539,7 @@ def tile_merge_pa_kernel(tc, x, w_c1, b_c1, w_q, w_k, w_v, bn_gamma, bn_beta, pr
                 j = slot_of(s, i)
                 pump_to(("k", s, j))
                 if i == 0:
-                    z = main.tile([P, 9, 512], F32, name="z", tag="z", bufs=3)
+                    z = main.tile([P, 9, 512], F32, name="z", tag="z", bufs=3, align_bytes=256)
                     zs[s] = z
                 nc.vector.tensor_tensor(out=zs[s][:, j, :], in0=q_sbs[s][:], in1=banks[("k", s, j)][:], op=ALU.mult)
 
@@ -605,7 +605,7 @@ def tile_merge_pa_kernel(tc, x, w_c1, b_c1, w_q, w_k, w_v, bn_gamma, bn_beta, pr
             for tok, s, slot in products(a)[i0:i1]:
                 pump_to(tok)
                 if s not in evs:
-                    ev = main.tile([P, 9, 512], F32, name="ev", tag="ev", bufs=2)
+                    ev = main.tile([P, 9, 512], F32, name="ev", tag="ev", bufs=2, align_bytes=256)
                     evs[s] = ev
                 nc.vector.tensor_tensor(out=evs[s][:, slot, :], in0=zs[s][:, slot, :], in1=banks[tok][:], op=ALU.mult)
 
@@ -703,17 +703,17 @@ def tile_merge_pa_kernel(tc, x, w_c1, b_c1, w_q, w_k, w_v, bn_gamma, bn_beta, pr
                 haar_from_turned(1)
                 halve(2, 2, late_sums[:])
                 haar_from_turned(3, 2)
-                g_v = weight_copies(W_V)
             if ok(s - 2):
                 weigh(s - 2, 0, 12)
             if s == 2:
                 quant_y(2)
             if s == 0:
+                g_v = weight_copies(W_V)
                 quant_ll(1)
                 add_bias_on_scalar(1)()
-                tree_in_halves(s, nothing, 0, lambda: quant_y(1))
+                tree_in_halves(s, lambda: quant_w(W_V, g_v), 0, lambda: quant_y(1))
             elif s == 1:
-                shift_by_max(s, (lambda: quant_ll(2), lambda: quant_w(W_V, g_v), nothing), 0, True)
+                tree_in_halves(s, nothing, 0, lambda: quant_ll(2))
                 scores(s + 1, 0, AHEAD)
             else:
                 tree_in_halves(s, (lambda: move_y(2)) if s == 2 else nothing, LAST_ON_VECTOR if s == STEPS - 1 else 0)
@@ -826,9 +826,9 @@ def tile_merge_pa_kernel(tc, x, w_c1, b_c1, w_q, w_k, w_v, bn_gamma, bn_beta, pr
 
         def normalise(ob):
             if ob < 3:
-                n = main.tile([P, NPIX], F32, name="n", tag="z", bufs=3)
+                n = main.tile([P, NPIX], F32, name="n", tag="z", bufs=3, align_bytes=256)
             else:
-                n = main.tile([P, NPIX], F32, name="n_last", tag="ev", bufs=2)
+                n = main.tile([P, NPIX], F32, name="n_last", tag="ev", bufs=2, align_bytes=256)
             ns[ob] = n
             if ob < 3:
                 normalise_images(ob, 0, NB)

@@ -132,6 +132,7 @@ def tile_merge_pa_kernel(tc, x, w_c1, b_c1, w_q, w_k, w_v, bn_gamma, bn_beta, pr
         neg_pivot = keep.tile([P, 4], F32, name="neg_pivot")
         one_minus_a = keep.tile([P, 1], F32, name="one_minus_a")
         gam_f = keep.tile([P, 4], F32, name="gam_f")
+        neg_beta = keep.tile([P, 4], F32, name="neg_beta")
         bias_full = keep.tile([P, ROW, 4], BF16, name="bias_full")
 
         ll = mid.tile([P, NPIX, 4], BF16, name="ll", align_bytes=64)
@@ -162,14 +163,14 @@ def tile_merge_pa_kernel(tc, x, w_c1, b_c1, w_q, w_k, w_v, bn_gamma, bn_beta, pr
         def ok(s):
             return 0 <= s < STEPS
 
-        def conv(dst, s, j, wi, start=True, stop=True):
-            window(dst, 2 * s + j // 3 - 1, j % 3, wi, start, stop)
+        def conv(dst, s, j, wi, start=True, stop=True, channels=slice(0, 512)):
+            window(dst, 2 * s + j // 3 - 1, j % 3, wi, start, stop, channels)
 
-        def window(dst, r, d, wi, start=True, stop=True):
+        def window(dst, r, d, wi, start=True, stop=True, channels=slice(0, 512)):
             c0 = ROW + ROW * r
             nc.tensor.matmul_mx(out=dst, lhsT=y_codes[d][:, c0:c0 + P].bitcast(FP8X4),
                                 lhsT_scale=y_scales[d][:, c0:c0 + P],
-                                rhs=w_codes[wi][:].bitcast(FP8X4), rhs_scale=w_scales[wi][:],
+                                rhs=w_codes[wi][:, channels].bitcast(FP8X4), rhs_scale=w_scales[wi][:, channels],
                                 start=start, stop=stop)
 
         def first_conv(bank, r):
@@ -198,12 +199,12 @@ def tile_merge_pa_kernel(tc, x, w_c1, b_c1, w_q, w_k, w_v, bn_gamma, bn_beta, pr
                 q_ps = psm.tile([P, 512], F32, name="q_ps", tag="k_ps", bufs=3)
                 conv(q_ps[:], s, 4, W_Q)
                 banks[tok] = q_ps
-            elif kind == "K":
-                k_ps = psm.tile([P, 512], F32, name="k_ps", tag="k_ps", bufs=3)
-                conv(k_ps[:], s, AROUND[j], W_K, True, False)
-                banks[("k", s, j)] = k_ps
-            elif kind == "k" and ("K", s, j) in done:
-                conv(banks[tok][:], s, CENTRE, W_KN, False, True)
+            elif kind == "b":
+                half_bank = psm.tile([P, 256], F32, name="k_half", tag=("k_ps" if j == 0 else ("num", "den")[s]), bufs=(3 if j == 0 else 1))
+                conv(half_bank[:], 0, AROUND[FIRST_SLOTS[s]], W_K, True, False, slice(256 * j, 256 * (j + 1)))
+                banks[tok] = half_bank
+            elif kind == "B":
+                conv(banks[("b", s, j)][:], 0, CENTRE, W_KN, False, True, slice(256 * j, 256 * (j + 1)))
             elif kind == "k":
                 if j == AHEAD and s >= FIRST_LENT:
                     k_ps = psm.tile([P, 512], F32, name="k_lent", tag="den", bufs=1)
@@ -352,7 +353,8 @@ def tile_merge_pa_kernel(tc, x, w_c1, b_c1, w_q, w_k, w_v, bn_gamma, bn_beta, pr
 
         pe_list = [("d", 0, i) for i in range(WARM_UP)] + [("w", W_C1, 0), ("w", W_C1, 1)] + on_pe(0) + [("w", W_Q, 0), ("w", W_Q, 1), ("c", 0, 0), ("c", 1, 0),
                                                                  ("w", W_K, 0), ("w", W_K, 1)] + on_pe(1)
-        pe_list += [("q", 0, 0)] + [("K", 0, j) for j in FIRST_SLOTS[0:2]] + [("k", 0, j) for j in FIRST_SLOTS[0:AHEAD]]
+        pe_list += [("q", 0, 0)] + [("b", 0, 0), ("B", 0, 0), ("b", 1, 0), ("B", 1, 0), ("b", 0, 1), ("b", 1, 1), ("B", 0, 1), ("B", 1, 1)]
+        pe_list += [("k", 0, j) for j in FIRST_SLOTS[2:AHEAD]]
         for s in range(STEPS + 2):
             a = s - 2
             if ok(s):
@@ -534,6 +536,15 @@ def tile_merge_pa_kernel(tc, x, w_c1, b_c1, w_q, w_k, w_v, bn_gamma, bn_beta, pr
             nc.scalar.copy(out=q_sb[:], in_=banks[("q", s, 0)][:])
             q_sbs[s] = q_sb
 
+        def first_scores():
+            z = main.tile([P, 9, 512], F32, name="z", tag="z", bufs=3, align_bytes=256)
+            zs[0] = z
+            for h in range(2):
+                for i in range(2):
+                    pump_to(("B", i, h))
+                    c = slice(256 * h, 256 * (h + 1))
+                    nc.vector.tensor_tensor(out=z[:, FIRST_SLOTS[i], c], in0=q_sbs[0][:, c], in1=banks[("b", i, h)][:], op=ALU.mult)
+
         def scores(s, j0, j1):
             for i in range(j0, j1):
                 j = slot_of(s, i)
@@ -639,6 +650,11 @@ def tile_merge_pa_kernel(tc, x, w_c1, b_c1, w_q, w_k, w_v, bn_gamma, bn_beta, pr
             if on_vector < 4:
                 nc.gpsimd.tensor_tensor(out=att[:, on_vector:4, cols], in0=num_sb[:], in1=rds[s][:, on_vector:4, :], op=ALU.mult)
 
+        def plain_sum(s, ob):
+            junk = main.tile([P, 2 * P], F32, name="junk_v", tag="junk_v", bufs=1)
+            nc.vector.tensor_scalar(out=junk[:], in0=att[:, ob, P * s:P * (s + 2)], scalar1=1.0, scalar2=None, op0=ALU.mult, op1=ALU.add,
+                                    accum_out=msums[:, 0, ob, s // 2:s // 2 + 1])
+
         def moments(s, first=0, end=8):
             cols = slice(P * s, P * (s + 2))
             for i in range(first, end):
@@ -659,9 +675,10 @@ def tile_merge_pa_kernel(tc, x, w_c1, b_c1, w_q, w_k, w_v, bn_gamma, bn_beta, pr
         haar_from_pe(0)
         quant_ll(0)
         g_q = weight_copies(W_Q)
+        quant_w_half(W_Q, g_q, 0)
         add_bias(0)
         add_bias(1)
-        quant_w(W_Q, g_q)
+        quant_w_half(W_Q, g_q, 1)
         g_k = weight_copies(W_K)
         quant_y(0)
         g_kn = main.tile([P, 2048], BF16, name="grouped_neg", tag="grouped", bufs=2, align_bytes=64)
@@ -685,7 +702,8 @@ def tile_merge_pa_kernel(tc, x, w_c1, b_c1, w_q, w_k, w_v, bn_gamma, bn_beta, pr
                 moments(2, 2 * part, 2 * part + 2)
 
         haar_on_vector(1, (2, 3), True)
-        scores(0, 0, AHEAD)
+        first_scores()
+        scores(0, 2, AHEAD)
         for s in range(STEPS):
             scores(s, AHEAD, scores_of(s))
             if ok(s - 3):
@@ -749,9 +767,10 @@ def tile_merge_pa_kernel(tc, x, w_c1, b_c1, w_q, w_k, w_v, bn_gamma, bn_beta, pr
                 one_over_den(s - 2)
             if s == 3:
                 nc.scalar.activation(out=neg_pivot[:], in_=att[:, :, 0], func=ACT.Copy, scale=-1.0)
-                nc.scalar.activation(out=msums[:, 0, :, PAIRS], in_=att[:, :, 0], func=ACT.Copy, scale=-2.0 * P)
+                nc.scalar.activation(out=msums[:, 0, :, PAIRS], in_=att[:, :, 0], func=ACT.Copy, scale=-4.0 * P)
                 nc.scalar.activation(out=one_minus_a[:], in_=a_bf[:], func=ACT.Identity, bias=1.0, scale=-1.0)
-                nc.scalar.copy(out=gam_f[:], in_=gam_bf[:])
+                nc.scalar.activation(out=gam_f[:], in_=gam_bf[:], func=ACT.Copy, scale=-1.0)
+                nc.scalar.activation(out=neg_beta[:], in_=bet_bf[:], func=ACT.Copy, scale=-1.0)
             if s == 6:
                 moments(2, 4, 8)
         lg_end = keep.tile([P, 4, 2, P], F32, name="lg_end")
@@ -761,7 +780,8 @@ def tile_merge_pa_kernel(tc, x, w_c1, b_c1, w_q, w_k, w_v, bn_gamma, bn_beta, pr
                                     in1=neg_m[:].unsqueeze(1).to_broadcast([P, g1 - g0, 512]), op=ALU.add)
         divide(STEPS - 3)
         exps(STEPS - 1, 0)
-        moments(STEPS - 4, 0, 3)
+        for ob in range(3):
+            moments(STEPS - 4, 2 * ob + 1, 2 * ob + 2)
         weigh(STEPS - 2, 0, 4)
         ev_sum = main.tile([P, 3, 512], F32, name="ev_sum", tag="t1", bufs=1)
         ev_sums.append(ev_sum)
@@ -773,8 +793,10 @@ def tile_merge_pa_kernel(tc, x, w_c1, b_c1, w_q, w_k, w_v, bn_gamma, bn_beta, pr
         weigh(STEPS - 1, 0, 6)
         ev7 = evs[STEPS - 1]
         nc.vector.tensor_tensor(out=ev7[:, 0:3, 0:128], in0=ev7[:, 0:3, 0:128], in1=ev7[:, 3:6, 0:128], op=ALU.add)
+        plain_sum(STEPS - 4, 0)
+        plain_sum(STEPS - 4, 1)
         root_of_last_den(STEPS - 1)
-        moments(STEPS - 4, 3, 6)
+        moments(STEPS - 4, 7, 8)
 
         last = slice(P * (STEPS - 2), NPIX)
         tot = keep.tile([P, 2, 4], F32, name="tot")
@@ -821,7 +843,7 @@ def tile_merge_pa_kernel(tc, x, w_c1, b_c1, w_q, w_k, w_v, bn_gamma, bn_beta, pr
             nc.scalar.activation(out=col(rstd, ob), in_=tot[:, 1, ob:ob + 1], func=ACT.Abs_reciprocal_sqrt, bias=col(dd, ob),
                                  scale=-1.0 / NPIX)
             nc.scalar.activation(out=col(gain, ob), in_=col(rstd, ob), func=ACT.Copy, scale=col(gam_f, ob))
-            nc.scalar.activation(out=col(shift, ob), in_=col(gain, ob), func=ACT.Identity, bias=col(bet_bf, ob),
+            nc.scalar.activation(out=col(shift, ob), in_=col(gain, ob), func=ACT.Identity, bias=col(neg_beta, ob),
                                  scale=col(neg_mean, ob))
 
         def normalise(ob):
@@ -830,8 +852,6 @@ def tile_merge_pa_kernel(tc, x, w_c1, b_c1, w_q, w_k, w_v, bn_gamma, bn_beta, pr
             else:
                 n = main.tile([P, NPIX], F32, name="n_last", tag="ev", bufs=2, align_bytes=256)
             ns[ob] = n
-            if ob < 3:
-                normalise_images(ob, 0, NB)
 
         def normalise_images(ob, b0, b1):
             nc.scalar.activation(out=ns[ob][:].rearrange("p (b y x) -> p b y x", b=NB, x=16)[:, b0:b1],
@@ -840,16 +860,25 @@ def tile_merge_pa_kernel(tc, x, w_c1, b_c1, w_q, w_k, w_v, bn_gamma, bn_beta, pr
 
         def minus_part(ob):
             neg = main.tile([P, NPIX], F32, name="neg", tag=("t1", "t2")[ob % 2], bufs=1)
-            nc.vector.tensor_scalar(out=neg[:], in0=ns[ob][:], scalar1=-1.0, scalar2=0.0, op0=ALU.mult, op1=ALU.max)
+            nc.scalar.activation(out=neg[:].rearrange("p (b y x) -> p b y x", b=NB, x=16),
+                                 in_=att[:, ob, :].rearrange("p (y b x) -> p b y x", b=NB, x=16),
+                                 func=ACT.Relu, bias=col(shift, ob), scale=col(gain, ob))
             negs[ob] = neg
+
+        def normalise_on_vector(ob, b0=0, b1=NB):
+            nc.vector.tensor_scalar(out=ns[ob][:].rearrange("p (b y x) -> p b y x", b=NB, x=16)[:, b0:b1],
+                                    in0=att[:, ob, :].rearrange("p (y b x) -> p b y x", b=NB, x=16)[:, b0:b1],
+                                    scalar1=col(gain, ob), scalar2=col(shift, ob), op0=ALU.mult, op1=ALU.add)
 
         def last_parts():
             neg = main.tile([P, NPIX], F32, name="neg_last", tag="t2", bufs=1)
             negs[3] = neg
             half = NPIX // 2
-            for h in range(2):
-                normalise_images(3, 2 * h, 2 * h + 2)
-                nc.scalar.activation(out=neg[:, half * h:half * (h + 1)], in_=ns[3][:, half * h:half * (h + 1)], func=ACT.Relu, scale=-1.0)
+            normalise_images(3, 0, 2)
+            nc.scalar.activation(out=neg[:, 0:half], in_=ns[3][:, 0:half], func=ACT.Relu)
+            nc.scalar.activation(out=neg[:, half:].rearrange("p (b y x) -> p b y x", b=2, x=16),
+                                 in_=att[:, 3, :].rearrange("p (y b x) -> p b y x", b=NB, x=16)[:, 2:4],
+                                 func=ACT.Relu, bias=col(shift, 3), scale=col(gain, 3))
 
         def prelu_and_store(ob, b0=0, b1=NB):
             if b0 == 0:
@@ -861,7 +890,7 @@ def tile_merge_pa_kernel(tc, x, w_c1, b_c1, w_q, w_k, w_v, bn_gamma, bn_beta, pr
                                                in0=negs[ob][:].rearrange("p (b f) -> p b f", b=NB)[:, b0:b1, src0:src0 + n_el],
                                                scalar=one_minus_a[:, 0:1],
                                                in1=ns[ob][:].rearrange("p (b f) -> p b f", b=NB)[:, b0:b1, src0:src0 + n_el],
-                                               op0=ALU.mult, op1=ALU.add)
+                                               op0=ALU.mult, op1=ALU.subtract)
             nc.sync.dma_start(out=out_v[:, ob, b0:b1], in_=res[:].rearrange("p (b f) -> p b f", b=NB)[:, b0:b1])
 
         B6 = STEPS - 2
@@ -870,37 +899,42 @@ def tile_merge_pa_kernel(tc, x, w_c1, b_c1, w_q, w_k, w_v, bn_gamma, bn_beta, pr
         divide_block(B7, 0)
         last_sum(0)
         last_squares(0)
-        moments(STEPS - 4, 6, 8)
+        plain_sum(STEPS - 4, 2)
         divide_block(B6, 1)
         divide_block(B7, 1)
+        plain_sum(STEPS - 4, 3)
         totals(0)
         statistics(0)
         last_sum(1)
         last_squares(1)
         normalise(0)
+        minus_part(0)
         divide_block(B6, 2)
-        totals(1)
         divide_block(B7, 2)
-        statistics(1)
+        normalise_on_vector(0)
+        totals(1)
         last_sum(2)
         last_squares(2)
-        normalise(1)
+        statistics(1)
         divide_block(B6, 3)
-        minus_part(0)
-        totals(2)
         divide_block(B7, 3)
-        statistics(2)
         last_sum(3)
         last_squares(3)
-        prelu_and_store(0)
-        normalise(2)
-        totals(3)
+        normalise(1)
         minus_part(1)
+        prelu_and_store(0)
+        totals(2)
+        statistics(2)
+        totals(3)
         statistics(3)
+        normalise(2)
+        minus_part(2)
+        normalise_on_vector(1)
         prelu_and_store(1)
+        normalise_on_vector(2)
         normalise(3)
         last_parts()
-        minus_part(2)
         prelu_and_store(2)
+        normalise_on_vector(3, 2, 4)
         prelu_and_store(3, 0, 2)
         prelu_and_store(3, 2, 4)

@@ -20,7 +20,7 @@ STEPS = 8
 BN_EPS = 1e-5
 BANK_DT = BF16
 AHEAD = 3
-SHARE_FROM = 1
+SHARE_FROM = 0
 WARM_UP = 4
 EARLY_FROM = 1
 FIRST_LENT = 2
@@ -30,6 +30,7 @@ LAST_ON_VECTOR = 3
 PIECES = ((0, 4), (4, 4), (8, 8))
 HAAR_ON_VECTOR = ((0, 0), (0, 1), (1, 2), (1, 3), (2, 2))
 TURNED = (0, 1)
+FIRST_IN_HALVES = (0, 3)
 W_C1, W_K, W_Q, W_V, W_KN = 0, 1, 2, 3, 4
 CENTRE = 4
 FIRST_SLOTS = (1, 6, 0, 2, 3, 4, 5, 7)
@@ -73,8 +74,9 @@ def tile_merge_pa_kernel(tc, x, w_c1, b_c1, w_q, w_k, w_v, bn_gamma, bn_beta, pr
         def load_x(pc):
             row0, nr = PIECES[pc]
             for b in range(NB):
-                nc.sync.dma_start(out=x_piece(pc, b),
-                                  in_=x[b].rearrange("(p j) h w -> p j (h w)", j=4)[:, :, ROW * row0:ROW * (row0 + nr)])
+                for j0, j1 in (((0, 2), (2, 4)) if (pc, b) == FIRST_IN_HALVES else ((0, 4),)):
+                    nc.sync.dma_start(out=x_piece(pc, b)[:, j0:j1],
+                                      in_=x[b].rearrange("(p j) h w -> p j (h w)", j=4)[:, j0:j1, ROW * row0:ROW * (row0 + nr)])
 
         bias_bf = keep.tile([P, 4], BF16, name="bias_bf")
         load_w(W_C1)
@@ -257,17 +259,18 @@ def tile_merge_pa_kernel(tc, x, w_c1, b_c1, w_q, w_k, w_v, bn_gamma, bn_beta, pr
                     for u in range(2):
                         nc.tensor.transpose(wT[:, rr, u, :], words[:, 2 * j + rr, u:256:2], ident[:])
                 banks[tok] = wT
-            elif kind == "h":
+            elif kind in ("h", "i"):
                 nr = PIECES[s][1]
                 taps = x_piece(s, j).rearrange("p j (i a x e) -> p j i a x e", a=2, x=16, e=2)
-                if j == NB - 1:
+                if j == NB - 1 and kind == "h":
                     hs = psm.tile([P, 512], F32, name="hs_last", tag="den", bufs=1)
                 else:
                     hs = psm.tile([P, 512], F32, name="hs", tag="v_ps", bufs=3)
-                nj = 2 if s == 2 else 4
+                j0 = 2 if kind == "i" else 0
+                nj = 2 if s == 2 or (s, j) == FIRST_IN_HALVES else 4
                 for n in range(4):
                     nc.tensor.matmul(out=hs[:, 0:16 * nj * nr].rearrange("p (j i x) -> p j i x", j=nj, x=16), lhsT=ident_bf[:],
-                                     rhs=taps[:, 0:nj, :, n // 2, :, n % 2], start=(n == 0), stop=(n == 3))
+                                     rhs=taps[:, j0:j0 + nj, :, n // 2, :, n % 2], start=(n == 0), stop=(n == 3))
                 banks[tok] = hs
             elif kind == "T":
                 xt = psm.tile([P, 8, P], BF16, name="xt", tag="v_ps", bufs=3)
@@ -349,7 +352,8 @@ def tile_merge_pa_kernel(tc, x, w_c1, b_c1, w_q, w_k, w_v, bn_gamma, bn_beta, pr
             return 4 * len(LAST_EXPS) if s == LAST else 36
 
         def on_pe(pc):
-            return [("h", pc, b) for b in range(NB) if (pc, b) not in HAAR_ON_VECTOR and (pc < 2 or b not in TURNED)]
+            toks = [("h", pc, b) for b in range(NB) if (pc, b) not in HAAR_ON_VECTOR and (pc < 2 or b not in TURNED)]
+            return toks + [("i", 0, FIRST_IN_HALVES[1])] if pc == FIRST_IN_HALVES[0] else toks
 
         pe_list = [("d", 0, i) for i in range(WARM_UP)] + [("w", W_C1, 0), ("w", W_C1, 1)] + on_pe(0) + [("w", W_Q, 0), ("w", W_Q, 1), ("c", 0, 0), ("c", 1, 0),
                                                                  ("w", W_K, 0), ("w", W_K, 1)] + on_pe(1)
@@ -392,9 +396,8 @@ def tile_merge_pa_kernel(tc, x, w_c1, b_c1, w_q, w_k, w_v, bn_gamma, bn_beta, pr
                 pe_list.extend([("k", s + 1, j) for j in range(AHEAD)])
             pe_list.extend(den_sums[18:])
             pe_list.extend(num_sums)
-            pe_list.extend(early)
-            if ok(s + 1):
-                pe_list.extend([("k", s + 1, AHEAD + j) for j in range(LATE)])
+            late_k = [("k", s + 1, AHEAD + j) for j in range(LATE)] if ok(s + 1) else []
+            pe_list.extend(late_k[:1] + early + late_k[1:])
         for ob in range(4):
             pe_list.extend([("G", STEPS - 2, 6 * ob + j) for j in range(6)])
             pe_list.extend([("G", STEPS - 1, 6 * ob + j) for j in range(3 if ob < 1 else 6)])
@@ -433,7 +436,15 @@ def tile_merge_pa_kernel(tc, x, w_c1, b_c1, w_q, w_k, w_v, bn_gamma, bn_beta, pr
         def haar_from_pe(pc):
             for tok in on_pe(pc):
                 pump_to(tok)
-                halve(pc, tok[2], banks[tok][:, 0:ROW * PIECES[pc][1]])
+                n = 2 * 16 * PIECES[pc][1]
+                if tok[0] == "i":
+                    nc.vector.tensor_scalar(out=ll_by_image[:, tok[2], 0:PIECES[pc][1], :, 2:4],
+                                            in0=banks[tok][:, 0:n].rearrange("p (j y x) -> p y x j", j=2, x=16), scalar1=0.5, scalar2=None,
+                                            op0=ALU.mult)
+                elif tok[1:] == FIRST_IN_HALVES:
+                    halve(pc, tok[2], banks[tok][:, 0:n], 0, 2)
+                else:
+                    halve(pc, tok[2], banks[tok][:, 0:2 * n])
 
         def haar_on_vector(pc, images, on_gpsimd=False, between=None):
             eng = nc.gpsimd if on_gpsimd else nc.vector
@@ -560,7 +571,7 @@ def tile_merge_pa_kernel(tc, x, w_c1, b_c1, w_q, w_k, w_v, bn_gamma, bn_beta, pr
             eng.tensor_tensor(out=z[:, g0:g1, :], in0=z[:, g0:g1, :], in1=ms[s][:].unsqueeze(1).to_broadcast([P, g1 - g0, 512]),
                               op=ALU.subtract)
 
-        def tree_in_halves(s, between, on_vector=0, before_m=None):
+        def tree_in_halves(s, between, on_vector=0, within=None):
             z = zs[s]
             halves = (slice(0, 256), slice(256, 512))
             n = scores_of(s) // 2
@@ -571,8 +582,8 @@ def tile_merge_pa_kernel(tc, x, w_c1, b_c1, w_q, w_k, w_v, bn_gamma, bn_beta, pr
             t2 = main.tile([P, 2, 512], F32, name="t2", tag="t2", bufs=1)
             for c in halves:
                 nc.vector.tensor_tensor(out=t2[:, 0:n // 2, c], in0=t1[:, 0:n // 2, c], in1=t1[:, n // 2:2 * (n // 2), c], op=ALU.max)
-            if before_m is not None:
-                before_m()
+                if within is not None and c == halves[0]:
+                    within()
             m = main.tile([P, 512], F32, name="m", tag="m")
             for c in halves:
                 other = t1[:, 2, c] if s == LAST else t2[:, 1, c]

@@ -21,6 +21,9 @@ BN_EPS = 1e-5
 BANK_DT = BF16
 AHEAD = 3
 SHARE_FROM = 0
+IDLE_STEP_1 = 4
+IDLE_STEP_2 = 4
+IDLE_HEAD = 2
 WARM_UP = 4
 EARLY_FROM = 1
 FIRST_LENT = 2
@@ -355,7 +358,7 @@ def tile_merge_pa_kernel(tc, x, w_c1, b_c1, w_q, w_k, w_v, bn_gamma, bn_beta, pr
             toks = [("h", pc, b) for b in range(NB) if (pc, b) not in HAAR_ON_VECTOR and (pc < 2 or b not in TURNED)]
             return toks + [("i", 0, FIRST_IN_HALVES[1])] if pc == FIRST_IN_HALVES[0] else toks
 
-        pe_list = [("d", 0, i) for i in range(WARM_UP)] + [("w", W_C1, 0), ("w", W_C1, 1)] + on_pe(0) + [("w", W_Q, 0), ("w", W_Q, 1), ("c", 0, 0), ("c", 1, 0),
+        pe_list = [("d", 0, i) for i in range(WARM_UP)] + [("w", W_C1, 0), ("w", W_C1, 1)] + [("d", 3, i) for i in range(IDLE_HEAD)] + on_pe(0) + [("w", W_Q, 0), ("w", W_Q, 1), ("c", 0, 0), ("c", 1, 0),
                                                                  ("w", W_K, 0), ("w", W_K, 1)] + on_pe(1)
         pe_list += [("q", 0, 0)] + [("b", 0, 0), ("B", 0, 0), ("b", 1, 0), ("B", 1, 0), ("b", 0, 1), ("b", 1, 1), ("B", 0, 1), ("B", 1, 1)]
         pe_list += [("k", 0, j) for j in FIRST_SLOTS[2:AHEAD]]
@@ -369,7 +372,7 @@ def tile_merge_pa_kernel(tc, x, w_c1, b_c1, w_q, w_k, w_v, bn_gamma, bn_beta, pr
                 pe_list.extend([("w", W_V, 0), ("w", W_V, 1)] + [("C", 1, t) for t in range(4)] + [("T", 0, 0), ("T", 0, 1), ("T", 1, 0)] + on_pe(2))
             if s == 1:
                 pe_list.extend([("T", 1, 1), ("H", 0, 0), ("T", 3, 1), ("H", 1, 0), ("H", 3, 0)])
-                pe_list.extend([("k", s + 1, j) for j in range(AHEAD)] + [("C", 2, t) for t in range(4)])
+                pe_list.extend([("k", s + 1, j) for j in range(AHEAD)] + [("d", 1, i) for i in range(IDLE_STEP_1)] + [("C", 2, t) for t in range(4)])
             vb = v_banks(a)[3 if a >= EARLY_FROM else 0:] if ok(a) else []
             early = v_banks(a + 1)[:3] if ok(a + 1) and a + 1 >= EARLY_FROM else []
             den_sums = [("F", a, i) for i in range(den_terms(a))] if ok(a) else []
@@ -390,7 +393,7 @@ def tile_merge_pa_kernel(tc, x, w_c1, b_c1, w_q, w_k, w_v, bn_gamma, bn_beta, pr
             else:
                 pe_list.extend(den_sums[:18] + vb)
             if s in LATE_Q:
-                pe_list.extend(den_sums[18:] + [("q", s + 1, 0)])
+                pe_list.extend(den_sums[18:] + ([("d", 2, i) for i in range(IDLE_STEP_2)] if s == 2 else []) + [("q", s + 1, 0)])
                 den_sums = den_sums[:18]
             if ok(s + 1) and s != 1:
                 pe_list.extend([("k", s + 1, j) for j in range(AHEAD)])

@@ -721,7 +721,7 @@ def tile_merge_pa_kernel(tc, x, w_c1, b_c1, w_q, w_k, w_v, bn_gamma, bn_beta, pr
         for s in range(STEPS):
             scores(s, AHEAD, scores_of(s))
             if ok(s - 3):
-                divide(s - 3, 2 if s < STEPS - 1 else 4)
+                divide(s - 3, 3 if s < STEPS - 1 else 4)
             if s == 1:
                 late_sums = haar_by_reduce(2, 2)
             if ok(s - 1):

@@ -40,6 +40,8 @@ FIRST_SLOTS = (1, 6, 0, 2, 3, 4, 5, 7)
 AROUND = (0, 1, 2, 3, 5, 6, 7, 8)
 OFFSET_OF_SLOT = AROUND + (CENTRE,)
 GROUPS = ((0, 3), (3, 6), (6, 8))
+TWO_GROUPS = ((0, 3), (3, 8))
+IN_TWO = (2, 3, 4, 5)
 LAST = STEPS - 1
 LATE_Q = (0, 2)
 Y_ROWS = 19
@@ -568,8 +570,11 @@ def tile_merge_pa_kernel(tc, x, w_c1, b_c1, w_q, w_k, w_v, bn_gamma, bn_beta, pr
                     zs[s] = z
                 nc.vector.tensor_tensor(out=zs[s][:, j, :], in0=q_sbs[s][:], in1=banks[("k", s, j)][:], op=ALU.mult)
 
+        def groups_of(s):
+            return TWO_GROUPS if s in IN_TWO else GROUPS
+
         def subtract(s, g, eng):
-            g0, g1 = GROUPS[g]
+            g0, g1 = groups_of(s)[g]
             z = zs[s]
             eng.tensor_tensor(out=z[:, g0:g1, :], in0=z[:, g0:g1, :], in1=ms[s][:].unsqueeze(1).to_broadcast([P, g1 - g0, 512]),
                               op=ALU.subtract)
@@ -592,7 +597,7 @@ def tile_merge_pa_kernel(tc, x, w_c1, b_c1, w_q, w_k, w_v, bn_gamma, bn_beta, pr
                 other = t1[:, 2, c] if s == LAST else t2[:, 1, c]
                 nc.vector.scalar_tensor_tensor(out=m[:, c], in0=t2[:, 0, c], scalar=0.0, in1=other, op0=ALU.max, op1=ALU.max)
             ms[s] = m
-            for g in range(len(GROUPS)):
+            for g in range(len(groups_of(s))):
                 if 3 * g < on_vector:
                     subtract(s, g, nc.vector)
                 elif on_vector == 0:
@@ -623,7 +628,7 @@ def tile_merge_pa_kernel(tc, x, w_c1, b_c1, w_q, w_k, w_v, bn_gamma, bn_beta, pr
                     nc.scalar.activation(out=z[:, 8, :], in_=ms[s][:], func=ACT.Exp, scale=-1.0, bias=math.log(3.0))
                 else:
                     nc.scalar.activation(out=z[:, 8, :], in_=ms[s][:], func=ACT.Exp, scale=-1.0)
-            g0, g1 = GROUPS[g]
+            g0, g1 = groups_of(s)[g]
             nc.scalar.activation(out=z[:, g0:g1, :], in_=z[:, g0:g1, :], func=ACT.Exp)
 
         def weigh(a, i0, i1):
@@ -771,13 +776,18 @@ def tile_merge_pa_kernel(tc, x, w_c1, b_c1, w_q, w_k, w_v, bn_gamma, bn_beta, pr
                 if s == STEPS - 1:
                     one_over_den(s - 2)
                 in_waits(s, 0)
-                exps(s - 1, 1)
+                if s - 1 not in IN_TWO:
+                    exps(s - 1, 1)
                 in_waits(s, 1)
+                if s - 1 in IN_TWO:
+                    one_over_den(s - 2)
+                    exps(s - 1, 1)
                 if s == STEPS - 1:
                     neg_m = main.tile([P, 512], F32, name="neg_m", tag="m")
                     nc.scalar.activation(out=neg_m[:], in_=ms[s][:], func=ACT.Copy, scale=-1.0)
-                exps(s - 1, 2)
-            if ok(s - 2) and s < STEPS - 1:
+                if s - 1 not in IN_TWO:
+                    exps(s - 1, 2)
+            if ok(s - 2) and s < STEPS - 1 and s - 1 not in IN_TWO:
                 one_over_den(s - 2)
             if s == 3:
                 nc.scalar.activation(out=neg_pivot[:], in_=att[:, :, 0], func=ACT.Copy, scale=-1.0)

@@ -22,7 +22,6 @@ BANK_DT = BF16
 AHEAD = 3
 SHARE_FROM = 0
 IDLE_STEP_1 = 4
-IDLE_STEP_2 = 4
 IDLE_HEAD = 2
 WARM_UP = 4
 EARLY_FROM = 1
@@ -41,7 +40,7 @@ AROUND = (0, 1, 2, 3, 5, 6, 7, 8)
 OFFSET_OF_SLOT = AROUND + (CENTRE,)
 GROUPS = ((0, 3), (3, 6), (6, 8))
 TWO_GROUPS = ((0, 3), (3, 8))
-IN_TWO = (2, 3, 4, 5)
+IN_TWO = (0, 1, 2, 3, 4, 5)
 LAST = STEPS - 1
 LATE_Q = (0, 2)
 Y_ROWS = 19
@@ -86,7 +85,7 @@ def tile_merge_pa_kernel(tc, x, w_c1, b_c1, w_q, w_k, w_v, bn_gamma, bn_beta, pr
         bias_bf = keep.tile([P, 4], BF16, name="bias_bf")
         load_w(W_C1)
         load_x(0)
-        nc.sync.dma_start(out=bias_bf[:], in_=b_c1.rearrange("(p t) -> p t", t=4))
+        nc.scalar.dma_start(out=bias_bf[:], in_=b_c1.rearrange("(p t) -> p t", t=4))
         load_w(W_Q, 2)
         load_w(W_K, 2)
         load_x(1)
@@ -395,12 +394,12 @@ def tile_merge_pa_kernel(tc, x, w_c1, b_c1, w_q, w_k, w_v, bn_gamma, bn_beta, pr
             else:
                 pe_list.extend(den_sums[:18] + vb)
             if s in LATE_Q:
-                pe_list.extend(den_sums[18:] + ([("d", 2, i) for i in range(IDLE_STEP_2)] if s == 2 else []) + [("q", s + 1, 0)])
+                pe_list.extend(den_sums[18:] + (num_sums[:18] if s == 2 else []) + [("q", s + 1, 0)])
                 den_sums = den_sums[:18]
             if ok(s + 1) and s != 1:
                 pe_list.extend([("k", s + 1, j) for j in range(AHEAD)])
             pe_list.extend(den_sums[18:])
-            pe_list.extend(num_sums)
+            pe_list.extend(num_sums[18:] if s == 2 else num_sums)
             late_k = [("k", s + 1, AHEAD + j) for j in range(LATE)] if ok(s + 1) else []
             pe_list.extend(late_k[:1] + early + late_k[1:])
         for ob in range(4):
@@ -756,7 +755,6 @@ def tile_merge_pa_kernel(tc, x, w_c1, b_c1, w_q, w_k, w_v, bn_gamma, bn_beta, pr
                 tree_in_halves(s, (lambda: move_y(2)) if s == 2 else nothing, LAST_ON_VECTOR if s == STEPS - 1 else 0)
                 if s == 2:
                     exps(1, 1)
-                    exps(1, 2)
                     q_copy(3)
                 if ok(s + 1):
                     scores(s + 1, 0, AHEAD)
@@ -770,7 +768,6 @@ def tile_merge_pa_kernel(tc, x, w_c1, b_c1, w_q, w_k, w_v, bn_gamma, bn_beta, pr
                 scores(1, 0, AHEAD)
             if s == 1:
                 exps(0, 1)
-                exps(0, 2)
                 add_bias_on_scalar(2)()
             elif ok(s - 1) and s != 2:
                 if s == STEPS - 1:
@@ -787,7 +784,7 @@ def tile_merge_pa_kernel(tc, x, w_c1, b_c1, w_q, w_k, w_v, bn_gamma, bn_beta, pr
                     nc.scalar.activation(out=neg_m[:], in_=ms[s][:], func=ACT.Copy, scale=-1.0)
                 if s - 1 not in IN_TWO:
                     exps(s - 1, 2)
-            if ok(s - 2) and s < STEPS - 1 and s - 1 not in IN_TWO:
+            if ok(s - 2) and s < STEPS - 1 and (s == 2 or s - 1 not in IN_TWO):
                 one_over_den(s - 2)
             if s == 3:
                 nc.scalar.activation(out=neg_pivot[:], in_=att[:, :, 0], func=ACT.Copy, scale=-1.0)

@@ -21,7 +21,7 @@ BN_EPS = 1e-5
 BANK_DT = BF16
 AHEAD = 3
 SHARE_FROM = 0
-IDLE_STEP_1 = 4
+IDLE_STEP_1 = 2
 IDLE_HEAD = 2
 WARM_UP = 4
 EARLY_FROM = 1
@@ -390,7 +390,7 @@ def tile_merge_pa_kernel(tc, x, w_c1, b_c1, w_q, w_k, w_v, bn_gamma, bn_beta, pr
                 vb = []
                 den_sums = []
             if ok(a) and a < EARLY_FROM:
-                pe_list.extend(vb[:3] + den_sums[:9] + vb[3:5] + den_sums[9:18] + vb[5:])
+                pe_list.extend(vb[:3] + den_sums[:9] + vb[3:7] + den_sums[9:18] + vb[7:])
             else:
                 pe_list.extend(den_sums[:18] + vb)
             if s in LATE_Q:

@@ -48,6 +48,8 @@ OWN_ROWS = 14
 INNER_ROWS = 16
 LAST_WINDOWS = ((INNER_ROWS, 0), (INNER_ROWS, 1), (INNER_ROWS, 2), (OWN_ROWS, 0), (OWN_ROWS, 2), (OWN_ROWS, 1))
 LAST_EXPS = (8, 0, 1, 2, 3, 4, 5)
+LEFT_OUT = 7
+CLIP = 32.0
 
 FLOPS = 4 * 2 * 512 * 512 * 1024
 
@@ -581,16 +583,18 @@ def tile_merge_pa_kernel(tc, x, w_c1, b_c1, w_q, w_k, w_v, bn_gamma, bn_beta, pr
         def tree_in_halves(s, between, on_vector=0, within=None):
             z = zs[s]
             halves = (slice(0, 256), slice(256, 512))
-            n = scores_of(s) // 2
-            t1 = main.tile([P, 4, 512], F32, name="t1", tag="t1", bufs=1)
+            t1 = main.tile([P, 3, 512], F32, name="t1", tag="t1", bufs=1)
             for c in halves:
-                nc.vector.tensor_tensor(out=t1[:, 0:n, c], in0=z[:, 0:n, c], in1=z[:, n:2 * n, c], op=ALU.max)
+                nc.vector.tensor_tensor(out=t1[:, :, c], in0=z[:, 0:3, c], in1=z[:, 3:6, c], op=ALU.max)
             between()
             t2 = main.tile([P, 2, 512], F32, name="t2", tag="t2", bufs=1)
             for c in halves:
-                nc.vector.tensor_tensor(out=t2[:, 0:n // 2, c], in0=t1[:, 0:n // 2, c], in1=t1[:, n // 2:2 * (n // 2), c], op=ALU.max)
-                if within is not None and c == halves[0]:
-                    within()
+                nc.vector.tensor_tensor(out=t2[:, 0, c], in0=t1[:, 0, c], in1=t1[:, 1, c], op=ALU.max)
+                if c == halves[0]:
+                    if within is not None:
+                        within()
+                    if s < LAST:
+                        nc.vector.tensor_tensor(out=t2[:, 1, :], in0=t1[:, 2, :], in1=z[:, 6, :], op=ALU.max)
             m = main.tile([P, 512], F32, name="m", tag="m")
             for c in halves:
                 other = t1[:, 2, c] if s == LAST else t2[:, 1, c]
@@ -628,7 +632,12 @@ def tile_merge_pa_kernel(tc, x, w_c1, b_c1, w_q, w_k, w_v, bn_gamma, bn_beta, pr
                 else:
                     nc.scalar.activation(out=z[:, 8, :], in_=ms[s][:], func=ACT.Exp, scale=-1.0)
             g0, g1 = groups_of(s)[g]
-            nc.scalar.activation(out=z[:, g0:g1, :], in_=z[:, g0:g1, :], func=ACT.Exp)
+            if s < LAST and g1 > LEFT_OUT:
+                nc.scalar.activation(out=z[:, LEFT_OUT, :], in_=z[:, LEFT_OUT, :], func=ACT.Relu, scale=-1.0, bias=CLIP)
+                nc.scalar.activation(out=z[:, g0:LEFT_OUT, :], in_=z[:, g0:LEFT_OUT, :], func=ACT.Exp)
+                nc.scalar.activation(out=z[:, LEFT_OUT, :], in_=z[:, LEFT_OUT, :], func=ACT.Exp, scale=-1.0, bias=CLIP)
+            else:
+                nc.scalar.activation(out=z[:, g0:g1, :], in_=z[:, g0:g1, :], func=ACT.Exp)
 
         def weigh(a, i0, i1):
             for tok, s, slot in products(a)[i0:i1]:

@@ -34,22 +34,22 @@ HAAR_ON_VECTOR = ((0, 0), (0, 1), (1, 2), (1, 3), (2, 2))
 TURNED = (0, 1)
 FIRST_IN_HALVES = (0, 3)
 W_C1, W_K, W_Q, W_V, W_KN = 0, 1, 2, 3, 4
-CENTRE = 4
-FIRST_SLOTS = (1, 6, 0, 2, 3, 4, 5, 7)
-AROUND = (0, 1, 2, 3, 5, 6, 7, 8)
-OFFSET_OF_SLOT = AROUND + (CENTRE,)
-GROUPS = ((0, 3), (3, 6), (6, 8))
-TWO_GROUPS = ((0, 3), (3, 8))
+INNER, OWN, OUTER = -1, 0, 1
+WINDOWS = ((INNER, 0), (INNER, 2), (OWN, 0), (OWN, 2), (OUTER, 0), (OUTER, 2), (OUTER, 1))
+SCORES = 7
+OUTWARDS = 6
+ITSELF = 7
+INWARDS = 8
+SHARED_FROM = 1
+GROUPS = ((0, 2), (2, 5), (5, 7))
+TWO_GROUPS = ((0, 2), (2, 7))
 IN_TWO = (0, 1, 2, 3, 4, 5)
-LAST = STEPS - 1
-LATE_Q = (0, 2)
-Y_ROWS = 19
-OWN_ROWS = 14
-INNER_ROWS = 16
-LAST_WINDOWS = ((INNER_ROWS, 0), (INNER_ROWS, 1), (INNER_ROWS, 2), (OWN_ROWS, 0), (OWN_ROWS, 2), (OWN_ROWS, 1))
-LAST_EXPS = (8, 0, 1, 2, 3, 4, 5)
-LEFT_OUT = 7
 CLIP = 32.0
+LAST = STEPS - 1
+Y_ROWS = 2 * (STEPS + 1)
+LAST_WINDOWS = ((INNER, 0), (INNER, 1), (INNER, 2), (OWN, 0), (OWN, 2), (OWN, 1))
+LAST_GROUPS = ((0, 3), (3, 6))
+LAST_EXPS = (7, 0, 1, 2, 3, 4, 5)
 
 FLOPS = 4 * 2 * 512 * 512 * 1024
 
@@ -80,9 +80,15 @@ def tile_merge_pa_kernel(tc, x, w_c1, b_c1, w_q, w_k, w_v, bn_gamma, bn_beta, pr
         def load_x(pc):
             row0, nr = PIECES[pc]
             for b in range(NB):
-                for j0, j1 in (((0, 2), (2, 4)) if (pc, b) == FIRST_IN_HALVES else ((0, 4),)):
-                    nc.sync.dma_start(out=x_piece(pc, b)[:, j0:j1],
-                                      in_=x[b].rearrange("(p j) h w -> p j (h w)", j=4)[:, j0:j1, ROW * row0:ROW * (row0 + nr)])
+                rows = x[b].rearrange("(p j) (r a) w -> p j r (a w)", j=4, a=2)
+                if pc == 0:
+                    for j0, j1 in (((0, 2), (2, 4)) if b == FIRST_IN_HALVES[1] else ((0, 4),)):
+                        nc.sync.dma_start(out=x_piece(pc, b)[:, j0:j1], in_=rows[:, j0:j1, 6:10].rearrange("p j r f -> p j (r f)"))
+                else:
+                    n = nr // 2
+                    for h, r in enumerate((8 - row0 // 2 - n, 8 + row0 // 2)):
+                        nc.sync.dma_start(out=x_piece(pc, b)[:, :, ROW * n * h:ROW * n * (h + 1)],
+                                          in_=rows[:, :, r:r + n].rearrange("p j r f -> p j (r f)"))
 
         bias_bf = keep.tile([P, 4], BF16, name="bias_bf")
         load_w(W_C1)
@@ -132,14 +138,16 @@ def tile_merge_pa_kernel(tc, x, w_c1, b_c1, w_q, w_k, w_v, bn_gamma, bn_beta, pr
             y_scales.append(yst)
 
         att = keep.tile([P, 4, NPIX], F32, name="att")
-        PAIRS = STEPS // 2
-        msums = keep.tile([P, 2, 4, PAIRS + 1], F32, name="msums")
-        nc.vector.memset(msums[:, :, :, PAIRS], 0.0)
-        nc.vector.tensor_scalar(out=msums[:, 1, :, PAIRS], in0=msums[:, 1, :, PAIRS], scalar1=NPIX * BN_EPS,
+        ENDS, CONSTANT = 4, 5
+        msums = keep.tile([P, 2, 4, 6], F32, name="msums")
+        nc.vector.memset(msums[:].rearrange("p k o c -> p (k o c)"), 0.0)
+        nc.vector.tensor_scalar(out=msums[:, 1, :, CONSTANT], in0=msums[:, 1, :, CONSTANT], scalar1=NPIX * BN_EPS,
                                 scalar2=None, op0=ALU.add)
         neg_pivot = keep.tile([P, 4], F32, name="neg_pivot")
         one_minus_a = keep.tile([P, 1], F32, name="one_minus_a")
         gam_f = keep.tile([P, 4], F32, name="gam_f")
+        gam_n = keep.tile([P, 4], F32, name="gam_n")
+        gam_pivot = keep.tile([P, 4], F32, name="gam_pivot")
         neg_beta = keep.tile([P, 4], F32, name="neg_beta")
         bias_full = keep.tile([P, ROW, 4], BF16, name="bias_full")
 
@@ -158,6 +166,7 @@ def tile_merge_pa_kernel(tc, x, w_c1, b_c1, w_q, w_k, w_v, bn_gamma, bn_beta, pr
                                     op=ALU.add)
         x_turned = {}
         zs = {}
+        ws = {}
         evs = {}
         nums = {}
         dens = {}
@@ -171,11 +180,8 @@ def tile_merge_pa_kernel(tc, x, w_c1, b_c1, w_q, w_k, w_v, bn_gamma, bn_beta, pr
         def ok(s):
             return 0 <= s < STEPS
 
-        def conv(dst, s, j, wi, start=True, stop=True, channels=slice(0, 512)):
-            window(dst, 2 * s + j // 3 - 1, j % 3, wi, start, stop, channels)
-
-        def window(dst, r, d, wi, start=True, stop=True, channels=slice(0, 512)):
-            c0 = ROW + ROW * r
+        def window(dst, place, d, wi, start=True, stop=True, channels=slice(0, 512)):
+            c0 = P * (place + 1)
             nc.tensor.matmul_mx(out=dst, lhsT=y_codes[d][:, c0:c0 + P].bitcast(FP8X4),
                                 lhsT_scale=y_scales[d][:, c0:c0 + P],
                                 rhs=w_codes[wi][:, channels].bitcast(FP8X4), rhs_scale=w_scales[wi][:, channels],
@@ -193,7 +199,7 @@ def tile_merge_pa_kernel(tc, x, w_c1, b_c1, w_q, w_k, w_v, bn_gamma, bn_beta, pr
         def add_up(dst, src, i):
             ob = i // 9
             j = i % 9
-            nc.tensor.matmul(out=dst[:, ob, :], lhsT=src[:, j, P * ob:P * (ob + 1)], rhs=to_ybx[:],
+            nc.tensor.matmul(out=dst[:, ob, :], lhsT=src(j)[:, P * ob:P * (ob + 1)], rhs=to_ybx[:],
                              is_transpose=True, start=(j == 0), stop=(j == 8))
 
         def last_bank(s, ob):
@@ -205,24 +211,27 @@ def tile_merge_pa_kernel(tc, x, w_c1, b_c1, w_q, w_k, w_v, bn_gamma, bn_beta, pr
             kind, s, j = tok
             if kind == "q":
                 q_ps = psm.tile([P, 512], F32, name="q_ps", tag="k_ps", bufs=3)
-                conv(q_ps[:], s, 4, W_Q)
+                window(q_ps[:], s, 1, W_Q)
                 banks[tok] = q_ps
             elif kind == "b":
                 half_bank = psm.tile([P, 256], F32, name="k_half", tag=("k_ps" if j == 0 else ("num", "den")[s]), bufs=(3 if j == 0 else 1))
-                conv(half_bank[:], 0, AROUND[FIRST_SLOTS[s]], W_K, True, False, slice(256 * j, 256 * (j + 1)))
+                window(half_bank[:], (OUTER, OWN)[s], 1, W_K, True, False, slice(256 * j, 256 * (j + 1)))
                 banks[tok] = half_bank
             elif kind == "B":
-                conv(banks[("b", s, j)][:], 0, CENTRE, W_KN, False, True, slice(256 * j, 256 * (j + 1)))
+                window(banks[("b", s, j)][:], (OWN, INNER)[s], 1, W_KN, False, True, slice(256 * j, 256 * (j + 1)))
             elif kind == "k":
-                if j == AHEAD and s >= FIRST_LENT:
+                if s >= FIRST_LENT and j == bank_order(s)[AHEAD]:
                     k_ps = psm.tile([P, 512], F32, name="k_lent", tag="den", bufs=1)
                 else:
                     k_ps = psm.tile([P, 512], F32, name="k_ps", tag="k_ps", bufs=3)
-                if s < LAST:
-                    conv(k_ps[:], s, AROUND[j], W_K, True, False)
-                    conv(k_ps[:], s, CENTRE, W_KN, False, True)
+                if s == LAST:
+                    window(k_ps[:], s + LAST_WINDOWS[j][0], LAST_WINDOWS[j][1], W_K)
+                elif j == INWARDS:
+                    window(k_ps[:], s, 1, W_K, True, False)
+                    window(k_ps[:], s + INNER, 1, W_KN, False, True)
                 else:
-                    window(k_ps[:], LAST_WINDOWS[j][0], LAST_WINDOWS[j][1], W_K, True, True)
+                    window(k_ps[:], s + WINDOWS[j][0], WINDOWS[j][1], W_K, True, False)
+                    window(k_ps[:], s, 1, W_KN, False, True)
                 banks[tok] = k_ps
             elif kind == "d":
                 if j == 0:
@@ -230,7 +239,7 @@ def tile_merge_pa_kernel(tc, x, w_c1, b_c1, w_q, w_k, w_v, bn_gamma, bn_beta, pr
                     banks["idle"] = idle
                 nc.tensor.matmul_mx(out=banks["idle"][:], lhsT=w_codes[W_KN][:, 0:P].bitcast(FP8X4), lhsT_scale=w_scales[W_KN][:, 0:P],
                                     rhs=w_codes[W_KN][:].bitcast(FP8X4), rhs_scale=w_scales[W_KN][:], start=True, stop=True)
-            elif kind in ("v", "u"):
+            elif kind in ("v", "u", "o"):
                 if tok in in_k_banks:
                     v_ps = psm.tile([P, 512], F32, name="v_in_k", tag="k_ps", bufs=3)
                 elif tok in lent_to_v:
@@ -294,7 +303,7 @@ def tile_merge_pa_kernel(tc, x, w_c1, b_c1, w_q, w_k, w_v, bn_gamma, bn_beta, pr
             elif kind == "F":
                 if j == 0:
                     if s == STEPS - 1:
-                        den = psm.tile([P, 4, P], F32, name="den_last", tag="num", bufs=1)
+                        den = psm.tile([P, 4, P], F32, name="den_last", tag="v_ps", bufs=3)
                     else:
                         den = psm.tile([P, 4, P], F32, name="den", tag="den", bufs=1)
                     dens[s] = den
@@ -303,7 +312,7 @@ def tile_merge_pa_kernel(tc, x, w_c1, b_c1, w_q, w_k, w_v, bn_gamma, bn_beta, pr
                     nc.tensor.matmul(out=dens[s][:, j // n, :], lhsT=zs[s][:, LAST_EXPS[j % n], P * (j // n):P * (j // n + 1)],
                                      rhs=to_ybx[:], is_transpose=True, start=(j % n == 0), stop=(j % n == n - 1))
                 else:
-                    add_up(dens[s], zs[s], j)
+                    add_up(dens[s], lambda i: exp_of(s, i), j)
             elif kind == "G" and s == STEPS - 2:
                 ob = j // 6
                 if j % 6 == 0:
@@ -321,22 +330,35 @@ def tile_merge_pa_kernel(tc, x, w_c1, b_c1, w_q, w_k, w_v, bn_gamma, bn_beta, pr
                 if j == 0:
                     num = psm.tile([P, 4, P], F32, name="num", tag="num", bufs=1)
                     nums[s] = num
-                add_up(nums[s], evs[s], j)
+                add_up(nums[s], lambda i: evs[s][:, i, :], j)
+
+        def exp_of(s, slot):
+            return ws[s][:] if slot == INWARDS else zs[s][:, slot, :]
+
+        def bank_order(s):
+            if s == LAST:
+                return tuple(range(len(LAST_WINDOWS)))
+            if s == 0:
+                return (OUTWARDS, INWARDS, 0, 1, 2, 3, 4, 5)
+            if s <= SHARED_FROM:
+                return (0, 1, 2, 3, INWARDS, 4, 5, OUTWARDS)
+            return (0, 1, 2, 3, 4, 5, OUTWARDS)
 
         def products(a):
             todo = []
             if a == LAST:
-                return [(("v", LAST_WINDOWS[j][0], LAST_WINDOWS[j][1]), a, j) for j in range(len(LAST_WINDOWS))]
+                return [(("v" if place == OWN else "u", a + place, d), a, j) for j, (place, d) in enumerate(LAST_WINDOWS)]
             if a <= SHARE_FROM:
-                todo.extend([(("u", 2 * a - 1, d), a, d) for d in range(3)])
-            todo.append((("v", 2 * a, 0), a, 3))
-            todo.append((("v", 2 * a, 2), a, 4))
-            todo.append((("v", 2 * a, 1), a, 8))
-            for d in range(3):
-                todo.append((("v", 2 * a + 1, d), a, 5 + d))
+                todo.extend([(("u", a - 1, d), a, slot) for d, slot in ((0, 0), (2, 1), (1, INWARDS))])
+            outer = [(("o", a + 1, d), a, slot) for d, slot in ((0, 4), (2, 5), (1, OUTWARDS))]
+            own = []
+            for d, slot, inner_slot in ((0, 2, 0), (2, 3, 1), (1, ITSELF, INWARDS)):
+                own.append((("v", a, d), a, slot))
                 if a + 1 < LAST and a >= SHARE_FROM:
-                    todo.append((("v", 2 * a + 1, d), a + 1, d))
-            return todo
+                    own.append((("v", a, d), a + 1, inner_slot))
+            if a == STEPS - 2:
+                return todo + outer[:2] + own[:2] + outer[2:] + own[2:]
+            return todo + outer + own
 
         def v_banks(a):
             toks = []
@@ -349,10 +371,7 @@ def tile_merge_pa_kernel(tc, x, w_c1, b_c1, w_q, w_k, w_v, bn_gamma, bn_beta, pr
         in_k_banks = v_banks(STEPS - 3)[3:] + v_banks(STEPS - 2)[3:] + v_banks(STEPS - 1)[3:]
 
         def scores_of(s):
-            return len(LAST_WINDOWS) if s == LAST else 8
-
-        def slot_of(s, i):
-            return FIRST_SLOTS[i] if s == 0 else i
+            return len(bank_order(s))
 
         def den_terms(s):
             return 4 * len(LAST_EXPS) if s == LAST else 36
@@ -364,18 +383,18 @@ def tile_merge_pa_kernel(tc, x, w_c1, b_c1, w_q, w_k, w_v, bn_gamma, bn_beta, pr
         pe_list = [("d", 0, i) for i in range(WARM_UP)] + [("w", W_C1, 0), ("w", W_C1, 1)] + [("d", 3, i) for i in range(IDLE_HEAD)] + on_pe(0) + [("w", W_Q, 0), ("w", W_Q, 1), ("c", 0, 0), ("c", 1, 0),
                                                                  ("w", W_K, 0), ("w", W_K, 1)] + on_pe(1)
         pe_list += [("q", 0, 0)] + [("b", 0, 0), ("B", 0, 0), ("b", 1, 0), ("B", 1, 0), ("b", 0, 1), ("b", 1, 1), ("B", 0, 1), ("B", 1, 1)]
-        pe_list += [("k", 0, j) for j in FIRST_SLOTS[2:AHEAD]]
+        pe_list += [("k", 0, j) for j in bank_order(0)[2:AHEAD]]
         for s in range(STEPS + 2):
             a = s - 2
             if ok(s):
-                pe_list.extend([("k", s, slot_of(s, j)) for j in range(AHEAD if s == 0 else AHEAD + LATE, scores_of(s))])
-            if ok(s + 1) and s not in LATE_Q:
+                pe_list.extend([("k", s, j) for j in bank_order(s)[AHEAD if s == 0 else AHEAD + LATE:]])
+            if ok(s + 1):
                 pe_list.append(("q", s + 1, 0))
             if s == 0:
                 pe_list.extend([("w", W_V, 0), ("w", W_V, 1)] + [("C", 1, t) for t in range(4)] + [("T", 0, 0), ("T", 0, 1), ("T", 1, 0)] + on_pe(2))
             if s == 1:
                 pe_list.extend([("T", 1, 1), ("H", 0, 0), ("T", 3, 1), ("H", 1, 0), ("H", 3, 0)])
-                pe_list.extend([("k", s + 1, j) for j in range(AHEAD)] + [("d", 1, i) for i in range(IDLE_STEP_1)] + [("C", 2, t) for t in range(4)])
+                pe_list.extend([("k", s + 1, j) for j in bank_order(s + 1)[:AHEAD]] + [("d", 1, i) for i in range(IDLE_STEP_1)] + [("C", 2, t) for t in range(4)])
             vb = v_banks(a)[3 if a >= EARLY_FROM else 0:] if ok(a) else []
             early = v_banks(a + 1)[:3] if ok(a + 1) and a + 1 >= EARLY_FROM else []
             den_sums = [("F", a, i) for i in range(den_terms(a))] if ok(a) else []
@@ -395,14 +414,11 @@ def tile_merge_pa_kernel(tc, x, w_c1, b_c1, w_q, w_k, w_v, bn_gamma, bn_beta, pr
                 pe_list.extend(vb[:3] + den_sums[:9] + vb[3:7] + den_sums[9:18] + vb[7:])
             else:
                 pe_list.extend(den_sums[:18] + vb)
-            if s in LATE_Q:
-                pe_list.extend(den_sums[18:] + (num_sums[:18] if s == 2 else []) + [("q", s + 1, 0)])
-                den_sums = den_sums[:18]
             if ok(s + 1) and s != 1:
-                pe_list.extend([("k", s + 1, j) for j in range(AHEAD)])
+                pe_list.extend([("k", s + 1, j) for j in bank_order(s + 1)[:AHEAD]])
             pe_list.extend(den_sums[18:])
-            pe_list.extend(num_sums[18:] if s == 2 else num_sums)
-            late_k = [("k", s + 1, AHEAD + j) for j in range(LATE)] if ok(s + 1) else []
+            pe_list.extend(num_sums)
+            late_k = [("k", s + 1, j) for j in bank_order(s + 1)[AHEAD:AHEAD + LATE]] if ok(s + 1) else []
             pe_list.extend(late_k[:1] + early + late_k[1:])
         for ob in range(4):
             pe_list.extend([("G", STEPS - 2, 6 * ob + j) for j in range(6)])
@@ -507,7 +523,7 @@ def tile_merge_pa_kernel(tc, x, w_c1, b_c1, w_q, w_k, w_v, bn_gamma, bn_beta, pr
         def add_bias(r):
             pump_to(("c", r, 0))
             for yy in range(2):
-                c0 = P * r + ROW * yy
+                c0 = ROW * (2, 0, 1, 3)[2 * r + yy]
                 nc.vector.tensor_tensor(out=y_mid[:, c0:c0 + ROW, :].rearrange("p (x b) t -> p x b t", b=NB),
                                         in0=banks[("c", r, 0)][:, :, ROW * yy:ROW * (yy + 1)].rearrange("p t (b x) -> p x b t", b=NB),
                                         in1=bias_full[:].rearrange("p (x b) t -> p x b t", b=NB), op=ALU.add)
@@ -518,30 +534,30 @@ def tile_merge_pa_kernel(tc, x, w_c1, b_c1, w_q, w_k, w_v, bn_gamma, bn_beta, pr
             by_slot = main.tile([P, 4, n], BF16, name="by_slot", tag="by_slot", bufs=1)
             for t in range(4):
                 pump_to(("C", pc, t))
-                nc.scalar.activation(out=by_slot[:, t, :].rearrange("p (y x b) -> p y x b", x=16, b=NB),
-                                     in_=banks[("C", pc, t)][:].rearrange("p (y b x) -> p y x b", x=16, b=NB), func=ACT.Identity,
-                                     bias=bias_bf[:, t:t + 1], scale=1.0)
+                to = by_slot[:, t, :].rearrange("p (i h x b) -> p h i x b", h=2, x=16, b=NB)
+                rows = banks[("C", pc, t)][:].rearrange("p (h i b x) -> p h i x b", h=2, x=16, b=NB)
+                for h, half in enumerate((rows[:, 0, ::-1], rows[:, 1])):
+                    nc.scalar.activation(out=to[:, h], in_=half, func=ACT.Identity, bias=bias_bf[:, t:t + 1], scale=1.0)
             return lambda: nc.scalar.copy(out=y_mid[:, c0:c0 + n, :], in_=by_slot[:].rearrange("p t n -> p n t"))
 
         def quant_y(pc):
             p0 = ROW * PIECES[pc][0]
             n = ROW * PIECES[pc][1]
-            nc.vector.quantize_mx(out=y_codes[1][:, p0:p0 + n].bitcast(FP8X4),
-                                  scales=y_scales[1][:, p0:p0 + n],
+            nc.vector.quantize_mx(out=y_codes[1][:, P + p0:P + p0 + n].bitcast(FP8X4),
+                                  scales=y_scales[1][:, P + p0:P + p0 + n],
                                   in_=y_mid[:].rearrange("p c j -> p (c j)")[:, 4 * p0:4 * (p0 + n)])
 
         code_rows = [t[:].rearrange("p (r c) -> p r c", c=ROW) for t in y_codes]
         scale_rows = [t[:].bitcast(I32).rearrange("p (r c) -> p r c", c=ROW // 4) for t in y_scales]
 
+        def turn_middle():
+            for rows in (code_rows[1], scale_rows[1]):
+                nc.vector.tensor_copy(out=rows[:, 0:2, :], in_=rows[:, 3:1:-1, :])
+
         def move_y(pc):
-            r0 = PIECES[pc][0]
-            r1 = r0 + PIECES[pc][1]
+            r0 = 2 + PIECES[pc][0] if pc > 0 else 0
+            r1 = 2 + PIECES[pc][0] + PIECES[pc][1]
             w = ROW // 4
-            if r1 == 16:
-                for rows in (code_rows[1], scale_rows[1]):
-                    nc.vector.tensor_copy(out=rows[:, 16:19:2, :], in_=rows[:, 0:2, :])
-                    nc.vector.tensor_copy(out=rows[:, 17, :], in_=rows[:, 14, :])
-                r1 = Y_ROWS
             nc.vector.tensor_copy(out=code_rows[0][:, r0:r1, NB:ROW], in_=code_rows[1][:, r0:r1, 0:ROW - NB])
             nc.vector.tensor_copy(out=code_rows[2][:, r0:r1, 0:ROW - NB], in_=code_rows[1][:, r0:r1, NB:ROW])
             nc.vector.tensor_copy(out=scale_rows[0][:, r0:r1, 1:w], in_=scale_rows[1][:, r0:r1, 0:w - 1])
@@ -553,26 +569,39 @@ def tile_merge_pa_kernel(tc, x, w_c1, b_c1, w_q, w_k, w_v, bn_gamma, bn_beta, pr
             nc.scalar.copy(out=q_sb[:], in_=banks[("q", s, 0)][:])
             q_sbs[s] = q_sb
 
+        def new_scores(s):
+            z = main.tile([P, 8, 512], F32, name="z", tag="z", bufs=3, align_bytes=256)
+            zs[s] = z
+
+        def new_inwards(s):
+            w = main.tile([P, 512], F32, name="w", tag="w", bufs=4, align_bytes=256)
+            ws[s] = w
+
         def first_scores():
-            z = main.tile([P, 9, 512], F32, name="z", tag="z", bufs=3, align_bytes=256)
-            zs[0] = z
+            new_scores(0)
+            new_inwards(0)
             for h in range(2):
                 for i in range(2):
                     pump_to(("B", i, h))
                     c = slice(256 * h, 256 * (h + 1))
-                    nc.vector.tensor_tensor(out=z[:, FIRST_SLOTS[i], c], in0=q_sbs[0][:, c], in1=banks[("b", i, h)][:], op=ALU.mult)
+                    nc.vector.tensor_tensor(out=exp_of(0, bank_order(0)[i])[:, c], in0=q_sbs[0][:, c], in1=banks[("b", i, h)][:], op=ALU.mult)
 
-        def scores(s, j0, j1):
-            for i in range(j0, j1):
-                j = slot_of(s, i)
+        def scores(s, i0, i1):
+            for i in range(i0, i1):
+                j = bank_order(s)[i]
                 pump_to(("k", s, j))
                 if i == 0:
-                    z = main.tile([P, 9, 512], F32, name="z", tag="z", bufs=3, align_bytes=256)
-                    zs[s] = z
-                nc.vector.tensor_tensor(out=zs[s][:, j, :], in0=q_sbs[s][:], in1=banks[("k", s, j)][:], op=ALU.mult)
+                    new_scores(s)
+                if j == INWARDS:
+                    new_inwards(s)
+                nc.vector.tensor_tensor(out=exp_of(s, j), in0=q_sbs[s][:], in1=banks[("k", s, j)][:], op=ALU.mult)
+
+        def scores_inwards(s):
+            new_inwards(s + 1)
+            nc.vector.tensor_tensor(out=ws[s + 1][:], in0=q_sbs[s + 1][:], in1=banks[("k", s, OUTWARDS)][:], op=ALU.mult)
 
         def groups_of(s):
-            return TWO_GROUPS if s in IN_TWO else GROUPS
+            return LAST_GROUPS if s == LAST else TWO_GROUPS if s in IN_TWO else GROUPS
 
         def subtract(s, g, eng):
             g0, g1 = groups_of(s)[g]
@@ -580,12 +609,13 @@ def tile_merge_pa_kernel(tc, x, w_c1, b_c1, w_q, w_k, w_v, bn_gamma, bn_beta, pr
             eng.tensor_tensor(out=z[:, g0:g1, :], in0=z[:, g0:g1, :], in1=ms[s][:].unsqueeze(1).to_broadcast([P, g1 - g0, 512]),
                               op=ALU.subtract)
 
-        def tree_in_halves(s, between, on_vector=0, within=None):
+        def tree_in_halves(s, between, on_vector=0, within=None, behind=None):
             z = zs[s]
             halves = (slice(0, 256), slice(256, 512))
             t1 = main.tile([P, 3, 512], F32, name="t1", tag="t1", bufs=1)
+            n = 2 if s == LAST else 3
             for c in halves:
-                nc.vector.tensor_tensor(out=t1[:, :, c], in0=z[:, 0:3, c], in1=z[:, 3:6, c], op=ALU.max)
+                nc.vector.tensor_tensor(out=t1[:, 0:n, c], in0=z[:, 0:n, c], in1=z[:, n:2 * n, c], op=ALU.max)
             between()
             t2 = main.tile([P, 2, 512], F32, name="t2", tag="t2", bufs=1)
             for c in halves:
@@ -597,47 +627,40 @@ def tile_merge_pa_kernel(tc, x, w_c1, b_c1, w_q, w_k, w_v, bn_gamma, bn_beta, pr
                         nc.vector.tensor_tensor(out=t2[:, 1, :], in0=t1[:, 2, :], in1=z[:, 6, :], op=ALU.max)
             m = main.tile([P, 512], F32, name="m", tag="m")
             for c in halves:
-                other = t1[:, 2, c] if s == LAST else t2[:, 1, c]
+                other = z[:, 4, c] if s == LAST else t2[:, 1, c]
                 nc.vector.scalar_tensor_tensor(out=m[:, c], in0=t2[:, 0, c], scalar=0.0, in1=other, op0=ALU.max, op1=ALU.max)
             ms[s] = m
+            if behind is not None:
+                behind()
             for g in range(len(groups_of(s))):
                 if 3 * g < on_vector:
                     subtract(s, g, nc.vector)
                 elif on_vector == 0:
                     subtract(s, g, nc.gpsimd)
-
-        def shift_by_max(s, between, on_vector=0, all_before_m=False):
-            z = zs[s]
-            t1 = main.tile([P, 4, 512], F32, name="t1", tag="t1", bufs=1)
-            nc.vector.tensor_tensor(out=t1[:], in0=z[:, 0:4, :], in1=z[:, 4:8, :], op=ALU.max)
-            between[0]()
-            t2 = main.tile([P, 2, 512], F32, name="t2", tag="t2", bufs=1)
-            nc.vector.tensor_tensor(out=t2[:], in0=t1[:, 0:2, :], in1=t1[:, 2:4, :], op=ALU.max)
-            between[1]()
-            if all_before_m:
-                between[2]()
-            m = main.tile([P, 512], F32, name="m", tag="m")
-            nc.vector.scalar_tensor_tensor(out=m[:], in0=t2[:, 0, :], scalar=0.0, in1=t2[:, 1, :], op0=ALU.max, op1=ALU.max)
-            ms[s] = m
-            if not all_before_m:
-                between[2]()
-            for g in range(len(GROUPS)):
-                subtract(s, g, nc.vector if 3 * g < on_vector else nc.gpsimd)
+                if g == 0 and s < LAST:
+                    nc.gpsimd.tensor_tensor(out=ws[s][:], in0=ws[s][:], in1=m[:], op=ALU.add)
 
         def exps(s, g):
             z = zs[s]
             if g == 0:
                 if s == LAST:
-                    nc.scalar.activation(out=z[:, 8, :], in_=ms[s][:], func=ACT.Exp, scale=-1.0, bias=math.log(3.0))
+                    nc.scalar.activation(out=z[:, ITSELF, :], in_=ms[s][:], func=ACT.Exp, scale=-1.0, bias=math.log(3.0))
                 else:
-                    nc.scalar.activation(out=z[:, 8, :], in_=ms[s][:], func=ACT.Exp, scale=-1.0)
+                    nc.scalar.activation(out=z[:, ITSELF, :], in_=ms[s][:], func=ACT.Exp, scale=-1.0)
             g0, g1 = groups_of(s)[g]
-            if s < LAST and g1 > LEFT_OUT:
-                nc.scalar.activation(out=z[:, LEFT_OUT, :], in_=z[:, LEFT_OUT, :], func=ACT.Relu, scale=-1.0, bias=CLIP)
-                nc.scalar.activation(out=z[:, g0:LEFT_OUT, :], in_=z[:, g0:LEFT_OUT, :], func=ACT.Exp)
-                nc.scalar.activation(out=z[:, LEFT_OUT, :], in_=z[:, LEFT_OUT, :], func=ACT.Exp, scale=-1.0, bias=CLIP)
+            if s == LAST and g1 == scores_of(s):
+                g1 -= 1
+                nc.scalar.activation(out=z[:, g1, :], in_=z[:, g1, :], func=ACT.Relu, scale=-1.0, bias=CLIP)
+                nc.scalar.activation(out=z[:, g0:g1, :], in_=z[:, g0:g1, :], func=ACT.Exp)
+                nc.scalar.activation(out=z[:, g1, :], in_=z[:, g1, :], func=ACT.Exp, scale=-1.0, bias=CLIP)
             else:
                 nc.scalar.activation(out=z[:, g0:g1, :], in_=z[:, g0:g1, :], func=ACT.Exp)
+            if g == 0 and ok(s + 2):
+                q_copy(s + 2)
+            if g == 0 and s < LAST:
+                w = ws[s]
+                nc.scalar.activation(out=w[:], in_=w[:], func=ACT.Relu, scale=1.0, bias=CLIP)
+                nc.scalar.activation(out=w[:], in_=w[:], func=ACT.Exp, scale=-1.0, bias=CLIP)
 
         def weigh(a, i0, i1):
             for tok, s, slot in products(a)[i0:i1]:
@@ -645,7 +668,7 @@ def tile_merge_pa_kernel(tc, x, w_c1, b_c1, w_q, w_k, w_v, bn_gamma, bn_beta, pr
                 if s not in evs:
                     ev = main.tile([P, 9, 512], F32, name="ev", tag="ev", bufs=2, align_bytes=256)
                     evs[s] = ev
-                nc.vector.tensor_tensor(out=evs[s][:, slot, :], in0=zs[s][:, slot, :], in1=banks[tok][:], op=ALU.mult)
+                nc.vector.tensor_tensor(out=evs[s][:, slot, :], in0=exp_of(s, slot), in1=banks[tok][:], op=ALU.mult)
 
         def log_den(s):
             pump_to(("F", s, 35))
@@ -653,9 +676,13 @@ def tile_merge_pa_kernel(tc, x, w_c1, b_c1, w_q, w_k, w_v, bn_gamma, bn_beta, pr
             nc.scalar.activation(out=lg[:], in_=dens[s][:], func=ACT.Abs_reciprocal_sqrt)
             lgs[s] = lg
 
+        def end_rows(s):
+            i = LAST - s
+            return slice(i, 4 - i, 3 - 2 * i)
+
         def root_of_last_den(s):
             pump_to(("F", s, den_terms(s) - 1))
-            nc.scalar.activation(out=lg_end[:, :, s - (STEPS - 2), :], in_=dens[s][:], func=ACT.Abs_reciprocal_sqrt)
+            nc.scalar.activation(out=lg_end[:, :, end_rows(s), :], in_=dens[s][:].rearrange("p o (h f) -> p o h f", h=2), func=ACT.Abs_reciprocal_sqrt)
 
         def exp_minus_log(s):
             rd = main.tile([P, 4, P], F32, name="rd", tag="rd")
@@ -666,31 +693,47 @@ def tile_merge_pa_kernel(tc, x, w_c1, b_c1, w_q, w_k, w_v, bn_gamma, bn_beta, pr
             log_den(s)
             exp_minus_log(s)
 
+        att_rows = att[:].rearrange("p o (y f) -> p o y f", f=ROW)
+        att_pairs = att[:].rearrange("p o (g n) -> p o g n", n=P)
+
+        def by_row(t):
+            return t.rearrange("p o (h f) -> p o h f", h=2)
+
+        def of_two_blocks(s, ob):
+            i = s // 2
+            return att_pairs[:, ob, 3 - i:5 + i:2 * i + 1, :]
+
         def divide(s, on_vector=4):
             pump_to(("G", s, 35))
-            cols = slice(P * s, P * (s + 1))
+            att_s = att_rows[:, :, 7 - s:9 + s:2 * s + 1, :]
             if on_vector < 4:
                 num_sb = main.tile([P, 4 - on_vector, P], F32, name="num_sb", tag="num_sb")
                 nc.scalar.copy(out=num_sb[:], in_=nums[s][:, on_vector:4, :])
-            nc.vector.tensor_tensor(out=att[:, 0:on_vector, cols], in0=nums[s][:, 0:on_vector, :], in1=rds[s][:, 0:on_vector, :],
-                                    op=ALU.mult)
-            if on_vector < 4:
-                nc.gpsimd.tensor_tensor(out=att[:, on_vector:4, cols], in0=num_sb[:], in1=rds[s][:, on_vector:4, :], op=ALU.mult)
-
-        def plain_sum(s, ob):
-            junk = main.tile([P, 2 * P], F32, name="junk_v", tag="junk_v", bufs=1)
-            nc.vector.tensor_scalar(out=junk[:], in0=att[:, ob, P * s:P * (s + 2)], scalar1=1.0, scalar2=None, op0=ALU.mult, op1=ALU.add,
-                                    accum_out=msums[:, 0, ob, s // 2:s // 2 + 1])
+            if on_vector == 4:
+                col_s = s // 2 + s % 2
+                num, rd = by_row(nums[s][:]), by_row(rds[s][:])
+                for ob in range(4):
+                    nc.vector.scalar_tensor_tensor(out=att_s[:, ob], in0=num[:, ob], scalar=1.0, in1=rd[:, ob], op0=ALU.mult, op1=ALU.mult,
+                                                   accum_out=msums[:, 0, ob, col_s:col_s + 1])
+            else:
+                nc.vector.tensor_tensor(out=att_s[:, 0:on_vector], in0=by_row(nums[s][:, 0:on_vector, :]), in1=by_row(rds[s][:, 0:on_vector, :]),
+                                        op=ALU.mult)
+                nc.gpsimd.tensor_tensor(out=att_s[:, on_vector:4], in0=by_row(num_sb[:]), in1=by_row(rds[s][:, on_vector:4, :]), op=ALU.mult)
 
         def moments(s, first=0, end=8):
-            cols = slice(P * s, P * (s + 2))
             for i in range(first, end):
                 ob = i // 2
                 kind = i % 2
-                junk = main.tile([P, 2 * P], F32, name="junk", tag="junk")
-                nc.scalar.activation(out=junk[:], in_=att[:, ob, cols], func=(ACT.Identity, ACT.Square)[kind],
+                junk = main.tile([P, 2, P], F32, name="junk", tag="junk")
+                nc.scalar.activation(out=junk[:], in_=of_two_blocks(s, ob), func=(ACT.Identity, ACT.Square)[kind],
                                      bias=neg_pivot[:, ob:ob + 1], scale=1.0,
                                      accum_out=msums[:, kind, ob, s // 2:s // 2 + 1])
+
+        def second_piece():
+            quant_y(1)
+            move_y(1)
+            after_moves = keep.tile([P, 1], I32, name="after_moves")
+            nc.gpsimd.tensor_copy(out=after_moves[:], in_=scale_rows[2][:, 2 + PIECES[1][0], 0:1])
 
         def nothing():
             return None
@@ -712,6 +755,7 @@ def tile_merge_pa_kernel(tc, x, w_c1, b_c1, w_q, w_k, w_v, bn_gamma, bn_beta, pr
         nc.vector.tensor_scalar(out=g_kn[:, 0:1024], in0=g_k[:, 0:1024], scalar1=-1.0, scalar2=None, op0=ALU.mult)
         nc.scalar.activation(out=g_kn[:, 1024:2048], in_=g_k[:, 1024:2048], func=ACT.Copy, scale=-1.0)
         quant_w_half(W_K, g_k, 0)
+        turn_middle()
         quant_w_half(W_KN, g_kn, 0)
         quant_w_half(W_K, g_k, 1)
         move_y(0)
@@ -739,8 +783,10 @@ def tile_merge_pa_kernel(tc, x, w_c1, b_c1, w_q, w_k, w_v, bn_gamma, bn_beta, pr
                 late_sums = haar_by_reduce(2, 2)
             if ok(s - 1):
                 exps(s - 1, 0)
-            if ok(s + 1) and s not in LATE_Q:
-                q_copy(s + 1)
+            if s == 2:
+                lay_out()
+            if s == 0:
+                q_copy(1)
             if s == 1:
                 turn_copies(1, (1,))
                 haar_from_turned(0)
@@ -748,15 +794,21 @@ def tile_merge_pa_kernel(tc, x, w_c1, b_c1, w_q, w_k, w_v, bn_gamma, bn_beta, pr
                 haar_from_turned(1)
                 halve(2, 2, late_sums[:])
                 haar_from_turned(3, 2)
+            if s == STEPS - 1:
+                moments(2, 4, 8)
             if ok(s - 2):
-                weigh(s - 2, 0, 12)
+                weigh(s - 2, 0, 3)
+            if SHARED_FROM <= s and s + 1 < LAST:
+                scores_inwards(s)
+            if ok(s - 2):
+                weigh(s - 2, 3, 12)
             if s == 2:
                 quant_y(2)
             if s == 0:
                 g_v = weight_copies(W_V)
                 quant_ll(1)
                 add_bias_on_scalar(1)()
-                tree_in_halves(s, lambda: quant_w(W_V, g_v), 0, lambda: quant_y(1))
+                tree_in_halves(s, lambda: quant_w(W_V, g_v), 0, None, second_piece)
             elif s == 1:
                 tree_in_halves(s, nothing, 0, lambda: quant_ll(2))
                 scores(s + 1, 0, AHEAD)
@@ -764,23 +816,22 @@ def tile_merge_pa_kernel(tc, x, w_c1, b_c1, w_q, w_k, w_v, bn_gamma, bn_beta, pr
                 tree_in_halves(s, (lambda: move_y(2)) if s == 2 else nothing, LAST_ON_VECTOR if s == STEPS - 1 else 0)
                 if s == 2:
                     exps(1, 1)
-                    q_copy(3)
                 if ok(s + 1):
                     scores(s + 1, 0, AHEAD)
             if s == 0:
-                q_copy(1)
                 turn_copies(0, (0, 1))
                 turn_copies(1, (0,))
                 pump_to(("h", 2, 3))
                 halve(2, 3, banks[("h", 2, 3)][:, 0:256], 0, 2)
-                move_y(1)
                 scores(1, 0, AHEAD)
             if s == 1:
                 exps(0, 1)
-                add_bias_on_scalar(2)()
+                lay_out = add_bias_on_scalar(2)
             elif ok(s - 1) and s != 2:
                 if s == STEPS - 1:
-                    one_over_den(s - 2)
+                    pump_to(("F", s - 2, 35))
+                    den_5 = main.tile([P, 4, P], F32, name="den_5", tag="lg")
+                    nc.scalar.copy(out=den_5[:], in_=dens[s - 2][:])
                 in_waits(s, 0)
                 if s - 1 not in IN_TWO:
                     exps(s - 1, 1)
@@ -796,22 +847,19 @@ def tile_merge_pa_kernel(tc, x, w_c1, b_c1, w_q, w_k, w_v, bn_gamma, bn_beta, pr
             if ok(s - 2) and s < STEPS - 1 and (s == 2 or s - 1 not in IN_TWO):
                 one_over_den(s - 2)
             if s == 3:
-                nc.scalar.activation(out=neg_pivot[:], in_=att[:, :, 0], func=ACT.Copy, scale=-1.0)
-                nc.scalar.activation(out=msums[:, 0, :, PAIRS], in_=att[:, :, 0], func=ACT.Copy, scale=-4.0 * P)
+                nc.scalar.activation(out=neg_pivot[:], in_=att_rows[:, :, 7, 0], func=ACT.Copy, scale=-1.0)
+                nc.scalar.activation(out=msums[:, 0, :, CONSTANT], in_=att_rows[:, :, 7, 0], func=ACT.Copy, scale=-4.0 * P)
                 nc.scalar.activation(out=one_minus_a[:], in_=a_bf[:], func=ACT.Identity, bias=1.0, scale=-1.0)
                 nc.scalar.activation(out=gam_f[:], in_=gam_bf[:], func=ACT.Copy, scale=-1.0)
+                nc.scalar.activation(out=gam_n[:], in_=gam_bf[:], func=ACT.Copy, scale=1.0 / NPIX)
                 nc.scalar.activation(out=neg_beta[:], in_=bet_bf[:], func=ACT.Copy, scale=-1.0)
-            if s == 6:
-                moments(2, 4, 8)
-        lg_end = keep.tile([P, 4, 2, P], F32, name="lg_end")
+                nc.gpsimd.tensor_tensor(out=gam_pivot[:], in0=gam_f[:], in1=neg_pivot[:], op=ALU.mult)
+        lg_end = keep.tile([P, 4, 4, ROW], F32, name="lg_end")
         z_last = zs[STEPS - 1]
-        for g0, g1 in GROUPS[1:2]:
+        for g0, g1 in LAST_GROUPS[1:]:
             nc.gpsimd.tensor_tensor(out=z_last[:, g0:g1, :], in0=z_last[:, g0:g1, :],
                                     in1=neg_m[:].unsqueeze(1).to_broadcast([P, g1 - g0, 512]), op=ALU.add)
-        divide(STEPS - 3)
         exps(STEPS - 1, 0)
-        for ob in range(3):
-            moments(STEPS - 4, 2 * ob + 1, 2 * ob + 2)
         weigh(STEPS - 2, 0, 4)
         ev_sum = main.tile([P, 3, 512], F32, name="ev_sum", tag="t1", bufs=1)
         ev_sums.append(ev_sum)
@@ -819,19 +867,22 @@ def tile_merge_pa_kernel(tc, x, w_c1, b_c1, w_q, w_k, w_v, bn_gamma, bn_beta, pr
         nc.gpsimd.tensor_tensor(out=ev_sum[:], in0=ev6[:, 0:3, :], in1=ev6[:, 3:6, :], op=ALU.add)
         weigh(STEPS - 2, 4, 6)
         exps(STEPS - 1, 1)
+        lg_5 = main.tile([P, 4, P], F32, name="lg_5", tag="lg")
+        nc.scalar.activation(out=lg_5[:], in_=den_5[:], func=ACT.Abs_reciprocal_sqrt)
+        lgs[STEPS - 3] = lg_5
+        exp_minus_log(STEPS - 3)
         root_of_last_den(STEPS - 2)
         weigh(STEPS - 1, 0, 6)
         ev7 = evs[STEPS - 1]
         nc.vector.tensor_tensor(out=ev7[:, 0:3, 0:128], in0=ev7[:, 0:3, 0:128], in1=ev7[:, 3:6, 0:128], op=ALU.add)
-        plain_sum(STEPS - 4, 0)
-        plain_sum(STEPS - 4, 1)
         root_of_last_den(STEPS - 1)
-        moments(STEPS - 4, 7, 8)
+        divide(STEPS - 3)
+        for ob in range(4):
+            moments(STEPS - 4, 2 * ob + 1, 2 * ob + 2)
 
-        last = slice(P * (STEPS - 2), NPIX)
         tot = keep.tile([P, 2, 4], F32, name="tot")
         dd = keep.tile([P, 4], F32, name="dd")
-        neg_mean = keep.tile([P, 4], F32, name="neg_mean")
+        gam_mean = keep.tile([P, 4], F32, name="gam_mean")
         rstd = keep.tile([P, 4], F32, name="rstd")
         gain = keep.tile([P, 4], F32, name="gain")
         shift = keep.tile([P, 4], F32, name="shift")
@@ -848,19 +899,20 @@ def tile_merge_pa_kernel(tc, x, w_c1, b_c1, w_q, w_k, w_v, bn_gamma, bn_beta, pr
         def divide_block(s, ob):
             pump_to(("G", s, 6 * ob + (2 if s == STEPS - 1 and ob < 1 else 5)))
             if ob not in part:
-                once = main.tile([P, 2, P], F32, name="once", tag="once")
+                once = main.tile([P, 4, ROW], F32, name="once", tag="once")
                 part[ob] = once
-            nc.vector.tensor_tensor(out=part[ob][:, s - (STEPS - 2), :], in0=nums[(s, ob)][:], in1=lg_end[:, ob, s - (STEPS - 2), :], op=ALU.mult)
+            nc.vector.tensor_tensor(out=part[ob][:, end_rows(s), :], in0=nums[(s, ob)][:].rearrange("p (h f) -> p h f", h=2),
+                                    in1=lg_end[:, ob, end_rows(s), :], op=ALU.mult)
 
         def last_sum(ob):
-            nc.vector.scalar_tensor_tensor(out=att[:, ob, last], in0=part[ob][:].rearrange("p s n -> p (s n)"), scalar=1.0,
-                                           in1=lg_end[:, ob].rearrange("p s n -> p (s n)"), op0=ALU.mult, op1=ALU.mult,
-                                           accum_out=msums[:, 0, ob, PAIRS - 1:PAIRS])
+            nc.vector.scalar_tensor_tensor(out=of_two_blocks(STEPS - 2, ob), in0=part[ob][:].rearrange("p (g r) f -> p g (r f)", g=2), scalar=1.0,
+                                           in1=lg_end[:, ob].rearrange("p (g r) f -> p g (r f)", g=2), op0=ALU.mult, op1=ALU.mult,
+                                           accum_out=msums[:, 0, ob, ENDS:ENDS + 1])
 
         def last_squares(ob):
-            junk = main.tile([P, 2 * P], F32, name="junk2", tag="junk2")
-            nc.scalar.activation(out=junk[:], in_=att[:, ob, last], func=ACT.Square, bias=col(neg_pivot, ob), scale=1.0,
-                                 accum_out=msums[:, 1, ob, PAIRS - 1:PAIRS])
+            junk = main.tile([P, 2, P], F32, name="junk2", tag="junk2")
+            nc.scalar.activation(out=junk[:], in_=of_two_blocks(STEPS - 2, ob), func=ACT.Square, bias=col(neg_pivot, ob), scale=1.0,
+                                 accum_out=msums[:, 1, ob, ENDS:ENDS + 1])
 
         def totals(ob):
             nc.vector.tensor_reduce(out=tot[:, :, ob:ob + 1], in_=msums[:, :, ob:ob + 1, :], axis=mybir.AxisListType.X, op=ALU.add)
@@ -868,13 +920,13 @@ def tile_merge_pa_kernel(tc, x, w_c1, b_c1, w_q, w_k, w_v, bn_gamma, bn_beta, pr
         def statistics(ob):
             nc.vector.scalar_tensor_tensor(out=col(dd, ob), in0=tot[:, 0, ob:ob + 1], scalar=1.0 / (NPIX * NPIX), in1=tot[:, 0, ob:ob + 1],
                                            op0=ALU.mult, op1=ALU.mult)
-            nc.vector.tensor_scalar(out=col(neg_mean, ob), in0=tot[:, 0, ob:ob + 1], scalar1=-1.0 / NPIX, scalar2=col(neg_pivot, ob),
+            nc.vector.tensor_scalar(out=col(gam_mean, ob), in0=tot[:, 0, ob:ob + 1], scalar1=col(gam_n, ob), scalar2=col(gam_pivot, ob),
                                     op0=ALU.mult, op1=ALU.add)
             nc.scalar.activation(out=col(rstd, ob), in_=tot[:, 1, ob:ob + 1], func=ACT.Abs_reciprocal_sqrt, bias=col(dd, ob),
                                  scale=-1.0 / NPIX)
             nc.scalar.activation(out=col(gain, ob), in_=col(rstd, ob), func=ACT.Copy, scale=col(gam_f, ob))
-            nc.scalar.activation(out=col(shift, ob), in_=col(gain, ob), func=ACT.Identity, bias=col(neg_beta, ob),
-                                 scale=col(neg_mean, ob))
+            nc.scalar.activation(out=col(shift, ob), in_=col(rstd, ob), func=ACT.Identity, bias=col(neg_beta, ob),
+                                 scale=col(gam_mean, ob))
 
         def normalise(ob):
             if ob < 3:
@@ -915,52 +967,47 @@ def tile_merge_pa_kernel(tc, x, w_c1, b_c1, w_q, w_k, w_v, bn_gamma, bn_beta, pr
                 res = mid.tile([P, NPIX], F32, name="res", tag=("ll", "y_mid", "res_c", "res_d")[ob], align_bytes=64)
                 ress[ob] = res
             res = ress[ob]
-            for src0, n_el, dst0 in ((0, 240, 16), (240, 16, 0)):
-                nc.vector.scalar_tensor_tensor(out=res[:].rearrange("p (b f) -> p b f", b=NB)[:, b0:b1, dst0:dst0 + n_el],
-                                               in0=negs[ob][:].rearrange("p (b f) -> p b f", b=NB)[:, b0:b1, src0:src0 + n_el],
-                                               scalar=one_minus_a[:, 0:1],
-                                               in1=ns[ob][:].rearrange("p (b f) -> p b f", b=NB)[:, b0:b1, src0:src0 + n_el],
-                                               op0=ALU.mult, op1=ALU.subtract)
+            images = slice(ROW * 4 * b0, ROW * 4 * b1)
+            nc.vector.scalar_tensor_tensor(out=res[:, images], in0=negs[ob][:, images], scalar=one_minus_a[:, 0:1], in1=ns[ob][:, images],
+                                           op0=ALU.mult, op1=ALU.subtract)
             nc.sync.dma_start(out=out_v[:, ob, b0:b1], in_=res[:].rearrange("p (b f) -> p b f", b=NB)[:, b0:b1])
 
         B6 = STEPS - 2
         B7 = STEPS - 1
         divide_block(B6, 0)
         divide_block(B7, 0)
+        divide_block(B6, 1)
         last_sum(0)
         last_squares(0)
-        plain_sum(STEPS - 4, 2)
-        divide_block(B6, 1)
         divide_block(B7, 1)
-        plain_sum(STEPS - 4, 3)
-        totals(0)
-        statistics(0)
+        divide_block(B6, 2)
         last_sum(1)
         last_squares(1)
+        divide_block(B7, 2)
+        totals(0)
+        divide_block(B6, 3)
+        statistics(0)
         normalise(0)
         minus_part(0)
-        divide_block(B6, 2)
-        divide_block(B7, 2)
-        normalise_on_vector(0)
-        totals(1)
         last_sum(2)
         last_squares(2)
-        statistics(1)
-        divide_block(B6, 3)
         divide_block(B7, 3)
+        totals(1)
+        normalise_on_vector(0)
+        statistics(1)
         last_sum(3)
         last_squares(3)
         normalise(1)
         minus_part(1)
-        prelu_and_store(0)
         totals(2)
+        prelu_and_store(0)
         statistics(2)
+        normalise_on_vector(1)
         totals(3)
-        statistics(3)
         normalise(2)
         minus_part(2)
-        normalise_on_vector(1)
         prelu_and_store(1)
+        statistics(3)
         normalise_on_vector(2)
         normalise(3)
         last_parts()

@@ -48,7 +48,7 @@ CLIP = 32.0
 LAST = STEPS - 1
 Y_ROWS = 2 * (STEPS + 1)
 LAST_WINDOWS = ((INNER, 0), (INNER, 1), (INNER, 2), (OWN, 0), (OWN, 2), (OWN, 1))
-LAST_GROUPS = ((0, 3), (3, 6))
+LAST_GROUPS = ((0, 4), (4, 6))
 LAST_EXPS = (7, 0, 1, 2, 3, 4, 5)
 
 FLOPS = 4 * 2 * 512 * 512 * 1024
@@ -325,7 +325,7 @@ def tile_merge_pa_kernel(tc, x, w_c1, b_c1, w_q, w_k, w_v, bn_gamma, bn_beta, pr
                 if j % 6 == 0:
                     last_bank(s, ob)
                 nc.tensor.matmul(out=nums[(s, ob)][:], lhsT=evs[s][:, j % 6, P * ob:P * (ob + 1)], rhs=to_ybx[:],
-                                 is_transpose=True, start=(j % 6 == 0), stop=(j % 6 == (2 if ob < 1 else 5)))
+                                 is_transpose=True, start=(j % 6 == 0), stop=(j % 6 == 5))
             else:
                 if j == 0:
                     num = psm.tile([P, 4, P], F32, name="num", tag="num", bufs=1)
@@ -422,7 +422,7 @@ def tile_merge_pa_kernel(tc, x, w_c1, b_c1, w_q, w_k, w_v, bn_gamma, bn_beta, pr
             pe_list.extend(late_k[:1] + early + late_k[1:])
         for ob in range(4):
             pe_list.extend([("G", STEPS - 2, 6 * ob + j) for j in range(6)])
-            pe_list.extend([("G", STEPS - 1, 6 * ob + j) for j in range(3 if ob < 1 else 6)])
+            pe_list.extend([("G", STEPS - 1, 6 * ob + j) for j in range(6)])
 
         done = set()
         pos = [0]
@@ -615,7 +615,7 @@ def tile_merge_pa_kernel(tc, x, w_c1, b_c1, w_q, w_k, w_v, bn_gamma, bn_beta, pr
             t1 = main.tile([P, 3, 512], F32, name="t1", tag="t1", bufs=1)
             n = 2 if s == LAST else 3
             for c in halves:
-                nc.vector.tensor_tensor(out=t1[:, 0:n, c], in0=z[:, 0:n, c], in1=z[:, n:2 * n, c], op=ALU.max)
+                nc.vector.tensor_tensor(out=t1[:, 0:n, c], in0=z[:, 0:n, c], in1=z[:, 6 - n:6, c] if s == LAST else z[:, 3:6, c], op=ALU.max)
             between()
             t2 = main.tile([P, 2, 512], F32, name="t2", tag="t2", bufs=1)
             for c in halves:
@@ -627,7 +627,7 @@ def tile_merge_pa_kernel(tc, x, w_c1, b_c1, w_q, w_k, w_v, bn_gamma, bn_beta, pr
                         nc.vector.tensor_tensor(out=t2[:, 1, :], in0=t1[:, 2, :], in1=z[:, 6, :], op=ALU.max)
             m = main.tile([P, 512], F32, name="m", tag="m")
             for c in halves:
-                other = z[:, 4, c] if s == LAST else t2[:, 1, c]
+                other = z[:, 2, c] if s == LAST else t2[:, 1, c]
                 nc.vector.scalar_tensor_tensor(out=m[:, c], in0=t2[:, 0, c], scalar=0.0, in1=other, op0=ALU.max, op1=ALU.max)
             ms[s] = m
             if behind is not None:
@@ -648,14 +648,14 @@ def tile_merge_pa_kernel(tc, x, w_c1, b_c1, w_q, w_k, w_v, bn_gamma, bn_beta, pr
                 else:
                     nc.scalar.activation(out=z[:, ITSELF, :], in_=ms[s][:], func=ACT.Exp, scale=-1.0)
             g0, g1 = groups_of(s)[g]
-            if s == LAST and g1 == scores_of(s):
+            if s == LAST and g == 0:
                 g1 -= 1
                 nc.scalar.activation(out=z[:, g1, :], in_=z[:, g1, :], func=ACT.Relu, scale=-1.0, bias=CLIP)
                 nc.scalar.activation(out=z[:, g0:g1, :], in_=z[:, g0:g1, :], func=ACT.Exp)
                 nc.scalar.activation(out=z[:, g1, :], in_=z[:, g1, :], func=ACT.Exp, scale=-1.0, bias=CLIP)
             else:
                 nc.scalar.activation(out=z[:, g0:g1, :], in_=z[:, g0:g1, :], func=ACT.Exp)
-            if g == 0 and ok(s + 2):
+            if g == 0 and s + 1 < 4:
                 q_copy(s + 2)
             if g == 0 and s < LAST:
                 w = ws[s]
@@ -781,6 +781,8 @@ def tile_merge_pa_kernel(tc, x, w_c1, b_c1, w_q, w_k, w_v, bn_gamma, bn_beta, pr
                 divide(s - 3, 3 if s < STEPS - 1 else 4)
             if s == 1:
                 late_sums = haar_by_reduce(2, 2)
+            if s >= 4 and ok(s + 1):
+                q_copy(s + 1)
             if ok(s - 1):
                 exps(s - 1, 0)
             if s == 2:
@@ -839,9 +841,6 @@ def tile_merge_pa_kernel(tc, x, w_c1, b_c1, w_q, w_k, w_v, bn_gamma, bn_beta, pr
                 if s - 1 in IN_TWO:
                     one_over_den(s - 2)
                     exps(s - 1, 1)
-                if s == STEPS - 1:
-                    neg_m = main.tile([P, 512], F32, name="neg_m", tag="m")
-                    nc.scalar.activation(out=neg_m[:], in_=ms[s][:], func=ACT.Copy, scale=-1.0)
                 if s - 1 not in IN_TWO:
                     exps(s - 1, 2)
             if ok(s - 2) and s < STEPS - 1 and (s == 2 or s - 1 not in IN_TWO):
@@ -858,7 +857,7 @@ def tile_merge_pa_kernel(tc, x, w_c1, b_c1, w_q, w_k, w_v, bn_gamma, bn_beta, pr
         z_last = zs[STEPS - 1]
         for g0, g1 in LAST_GROUPS[1:]:
             nc.gpsimd.tensor_tensor(out=z_last[:, g0:g1, :], in0=z_last[:, g0:g1, :],
-                                    in1=neg_m[:].unsqueeze(1).to_broadcast([P, g1 - g0, 512]), op=ALU.add)
+                                    in1=ms[LAST][:].unsqueeze(1).to_broadcast([P, g1 - g0, 512]), op=ALU.subtract)
         exps(STEPS - 1, 0)
         weigh(STEPS - 2, 0, 4)
         ev_sum = main.tile([P, 3, 512], F32, name="ev_sum", tag="t1", bufs=1)
@@ -873,12 +872,10 @@ def tile_merge_pa_kernel(tc, x, w_c1, b_c1, w_q, w_k, w_v, bn_gamma, bn_beta, pr
         exp_minus_log(STEPS - 3)
         root_of_last_den(STEPS - 2)
         weigh(STEPS - 1, 0, 6)
-        ev7 = evs[STEPS - 1]
-        nc.vector.tensor_tensor(out=ev7[:, 0:3, 0:128], in0=ev7[:, 0:3, 0:128], in1=ev7[:, 3:6, 0:128], op=ALU.add)
         root_of_last_den(STEPS - 1)
         divide(STEPS - 3)
-        for ob in range(4):
-            moments(STEPS - 4, 2 * ob + 1, 2 * ob + 2)
+        moments(STEPS - 4, 1, 2)
+        moments(STEPS - 4, 3, 4)
 
         tot = keep.tile([P, 2, 4], F32, name="tot")
         dd = keep.tile([P, 4], F32, name="dd")
@@ -897,7 +894,7 @@ def tile_merge_pa_kernel(tc, x, w_c1, b_c1, w_q, w_k, w_v, bn_gamma, bn_beta, pr
         part = {}
 
         def divide_block(s, ob):
-            pump_to(("G", s, 6 * ob + (2 if s == STEPS - 1 and ob < 1 else 5)))
+            pump_to(("G", s, 6 * ob + 5))
             if ob not in part:
                 once = main.tile([P, 4, ROW], F32, name="once", tag="once")
                 part[ob] = once
@@ -947,6 +944,11 @@ def tile_merge_pa_kernel(tc, x, w_c1, b_c1, w_q, w_k, w_v, bn_gamma, bn_beta, pr
                                  func=ACT.Relu, bias=col(shift, ob), scale=col(gain, ob))
             negs[ob] = neg
 
+        def minus_part_on_vector(ob):
+            neg = main.tile([P, NPIX], F32, name="neg_v", tag=("t1", "t2")[ob % 2], bufs=1)
+            nc.vector.tensor_scalar(out=neg[:], in0=ns[ob][:], scalar1=0.0, scalar2=None, op0=ALU.max)
+            negs[ob] = neg
+
         def normalise_on_vector(ob, b0=0, b1=NB):
             nc.vector.tensor_scalar(out=ns[ob][:].rearrange("p (b y x) -> p b y x", b=NB, x=16)[:, b0:b1],
                                     in0=att[:, ob, :].rearrange("p (y b x) -> p b y x", b=NB, x=16)[:, b0:b1],
@@ -982,18 +984,20 @@ def tile_merge_pa_kernel(tc, x, w_c1, b_c1, w_q, w_k, w_v, bn_gamma, bn_beta, pr
         divide_block(B7, 1)
         divide_block(B6, 2)
         last_sum(1)
+        moments(STEPS - 4, 5, 6)
         last_squares(1)
         divide_block(B7, 2)
         totals(0)
         divide_block(B6, 3)
         statistics(0)
         normalise(0)
-        minus_part(0)
         last_sum(2)
+        moments(STEPS - 4, 7, 8)
         last_squares(2)
         divide_block(B7, 3)
         totals(1)
         normalise_on_vector(0)
+        minus_part_on_vector(0)
         statistics(1)
         last_sum(3)
         last_squares(3)

@@ -43,7 +43,7 @@ INWARDS = 8
 SHARED_FROM = 1
 GROUPS = ((0, 2), (2, 5), (5, 7))
 TWO_GROUPS = ((0, 2), (2, 7))
-IN_TWO = (0, 1, 2, 3, 4, 5)
+IN_TWO = (0, 1, 2, 3, 4, 5, 6)
 CLIP = 32.0
 LAST = STEPS - 1
 Y_ROWS = 2 * (STEPS + 1)
@@ -138,16 +138,14 @@ def tile_merge_pa_kernel(tc, x, w_c1, b_c1, w_q, w_k, w_v, bn_gamma, bn_beta, pr
             y_scales.append(yst)
 
         att = keep.tile([P, 4, NPIX], F32, name="att")
-        ENDS, CONSTANT = 4, 5
-        msums = keep.tile([P, 2, 4, 6], F32, name="msums")
-        nc.vector.memset(msums[:].rearrange("p k o c -> p (k o c)"), 0.0)
-        nc.vector.tensor_scalar(out=msums[:, 1, :, CONSTANT], in0=msums[:, 1, :, CONSTANT], scalar1=NPIX * BN_EPS,
-                                scalar2=None, op0=ALU.add)
+        msums = keep.tile([P, 2, 4, 2], F32, name="msums")
+        bn_parts = keep.tile([P, 4, 7, 3], F32, name="bn_parts")
+        first_four = keep.tile([P, 4, 2], F32, name="first_four")
+        nc.vector.memset(bn_parts[:, :, 0, 0], 4.0 * P)
         neg_pivot = keep.tile([P, 4], F32, name="neg_pivot")
         one_minus_a = keep.tile([P, 1], F32, name="one_minus_a")
         gam_f = keep.tile([P, 4], F32, name="gam_f")
-        gam_n = keep.tile([P, 4], F32, name="gam_n")
-        gam_pivot = keep.tile([P, 4], F32, name="gam_pivot")
+        gam_p = keep.tile([P, 4], F32, name="gam_p")
         neg_beta = keep.tile([P, 4], F32, name="neg_beta")
         bias_full = keep.tile([P, ROW, 4], BF16, name="bias_full")
 
@@ -671,21 +669,13 @@ def tile_merge_pa_kernel(tc, x, w_c1, b_c1, w_q, w_k, w_v, bn_gamma, bn_beta, pr
                 nc.vector.tensor_tensor(out=evs[s][:, slot, :], in0=exp_of(s, slot), in1=banks[tok][:], op=ALU.mult)
 
         def log_den(s):
-            pump_to(("F", s, 35))
-            lg = main.tile([P, 4, P], F32, name="lg", tag="lg")
+            pump_to(("F", s, den_terms(s) - 1))
+            lg = main.tile([P, 4, P], F32, name="lg", tag="lg", bufs=4)
             nc.scalar.activation(out=lg[:], in_=dens[s][:], func=ACT.Abs_reciprocal_sqrt)
             lgs[s] = lg
 
-        def end_rows(s):
-            i = LAST - s
-            return slice(i, 4 - i, 3 - 2 * i)
-
-        def root_of_last_den(s):
-            pump_to(("F", s, den_terms(s) - 1))
-            nc.scalar.activation(out=lg_end[:, :, end_rows(s), :], in_=dens[s][:].rearrange("p o (h f) -> p o h f", h=2), func=ACT.Abs_reciprocal_sqrt)
-
         def exp_minus_log(s):
-            rd = main.tile([P, 4, P], F32, name="rd", tag="rd")
+            rd = main.tile([P, 4, P], F32, name="rd", tag="rd", bufs=3)
             nc.scalar.activation(out=rd[:], in_=lgs[s][:], func=ACT.Square)
             rds[s] = rd
 
@@ -709,16 +699,25 @@ def tile_merge_pa_kernel(tc, x, w_c1, b_c1, w_q, w_k, w_v, bn_gamma, bn_beta, pr
             if on_vector < 4:
                 num_sb = main.tile([P, 4 - on_vector, P], F32, name="num_sb", tag="num_sb")
                 nc.scalar.copy(out=num_sb[:], in_=nums[s][:, on_vector:4, :])
-            if on_vector == 4:
-                col_s = s // 2 + s % 2
-                num, rd = by_row(nums[s][:]), by_row(rds[s][:])
-                for ob in range(4):
-                    nc.vector.scalar_tensor_tensor(out=att_s[:, ob], in0=num[:, ob], scalar=1.0, in1=rd[:, ob], op0=ALU.mult, op1=ALU.mult,
-                                                   accum_out=msums[:, 0, ob, col_s:col_s + 1])
-            else:
-                nc.vector.tensor_tensor(out=att_s[:, 0:on_vector], in0=by_row(nums[s][:, 0:on_vector, :]), in1=by_row(rds[s][:, 0:on_vector, :]),
-                                        op=ALU.mult)
+            nc.vector.tensor_tensor(out=att_s[:, 0:on_vector], in0=by_row(nums[s][:, 0:on_vector, :]), in1=by_row(rds[s][:, 0:on_vector, :]),
+                                    op=ALU.mult)
+            if on_vector < 4:
                 nc.gpsimd.tensor_tensor(out=att_s[:, on_vector:4], in0=by_row(num_sb[:]), in1=by_row(rds[s][:, on_vector:4, :]), op=ALU.mult)
+
+        def block_stats(s, ob):
+            i = 1 + 2 * (s - 4)
+            nc.vector.bn_stats(out=bn_parts[:, ob, i:i + 2, :].rearrange("p g i -> p (g i)"),
+                               in_=of_two_blocks(s, ob) if s == STEPS - 2 else att_rows[:, ob, 7 - s:9 + s:2 * s + 1, :])
+
+        def first_part():
+            half = keep.tile([P, 2, 4], F32, name="half")
+            mean = keep.tile([P, 4], F32, name="mean")
+            squared = keep.tile([P, 4], F32, name="squared")
+            nc.gpsimd.tensor_tensor(out=half[:], in0=msums[:, :, :, 0], in1=msums[:, :, :, 1], op=ALU.add)
+            nc.gpsimd.tensor_scalar(out=mean[:], in0=half[:, 0, :], scalar1=0.25 / P, scalar2=0.0, op0=ALU.mult, op1=ALU.add)
+            nc.gpsimd.tensor_tensor(out=squared[:], in0=half[:, 0, :], in1=mean[:], op=ALU.mult)
+            nc.gpsimd.tensor_tensor(out=first_four[:, :, 0], in0=mean[:], in1=neg_pivot[:], op=ALU.subtract)
+            nc.gpsimd.tensor_tensor(out=first_four[:, :, 1], in0=half[:, 1, :], in1=squared[:], op=ALU.subtract)
 
         def moments(s, first=0, end=8):
             for i in range(first, end):
@@ -832,14 +831,15 @@ def tile_merge_pa_kernel(tc, x, w_c1, b_c1, w_q, w_k, w_v, bn_gamma, bn_beta, pr
             elif ok(s - 1) and s != 2:
                 if s == STEPS - 1:
                     pump_to(("F", s - 2, 35))
-                    den_5 = main.tile([P, 4, P], F32, name="den_5", tag="lg")
+                    den_5 = main.tile([P, 4, P], F32, name="den_5", tag="lg", bufs=4)
                     nc.scalar.copy(out=den_5[:], in_=dens[s - 2][:])
                 in_waits(s, 0)
                 if s - 1 not in IN_TWO:
                     exps(s - 1, 1)
                 in_waits(s, 1)
                 if s - 1 in IN_TWO:
-                    one_over_den(s - 2)
+                    if s < STEPS - 1:
+                        one_over_den(s - 2)
                     exps(s - 1, 1)
                 if s - 1 not in IN_TWO:
                     exps(s - 1, 2)
@@ -847,13 +847,10 @@ def tile_merge_pa_kernel(tc, x, w_c1, b_c1, w_q, w_k, w_v, bn_gamma, bn_beta, pr
                 one_over_den(s - 2)
             if s == 3:
                 nc.scalar.activation(out=neg_pivot[:], in_=att_rows[:, :, 7, 0], func=ACT.Copy, scale=-1.0)
-                nc.scalar.activation(out=msums[:, 0, :, CONSTANT], in_=att_rows[:, :, 7, 0], func=ACT.Copy, scale=-4.0 * P)
                 nc.scalar.activation(out=one_minus_a[:], in_=a_bf[:], func=ACT.Identity, bias=1.0, scale=-1.0)
                 nc.scalar.activation(out=gam_f[:], in_=gam_bf[:], func=ACT.Copy, scale=-1.0)
-                nc.scalar.activation(out=gam_n[:], in_=gam_bf[:], func=ACT.Copy, scale=1.0 / NPIX)
+                nc.scalar.activation(out=gam_p[:], in_=gam_bf[:], func=ACT.Copy, scale=1.0)
                 nc.scalar.activation(out=neg_beta[:], in_=bet_bf[:], func=ACT.Copy, scale=-1.0)
-                nc.gpsimd.tensor_tensor(out=gam_pivot[:], in0=gam_f[:], in1=neg_pivot[:], op=ALU.mult)
-        lg_end = keep.tile([P, 4, 4, ROW], F32, name="lg_end")
         z_last = zs[STEPS - 1]
         for g0, g1 in LAST_GROUPS[1:]:
             nc.gpsimd.tensor_tensor(out=z_last[:, g0:g1, :], in0=z_last[:, g0:g1, :],
@@ -866,19 +863,21 @@ def tile_merge_pa_kernel(tc, x, w_c1, b_c1, w_q, w_k, w_v, bn_gamma, bn_beta, pr
         nc.gpsimd.tensor_tensor(out=ev_sum[:], in0=ev6[:, 0:3, :], in1=ev6[:, 3:6, :], op=ALU.add)
         weigh(STEPS - 2, 4, 6)
         exps(STEPS - 1, 1)
-        lg_5 = main.tile([P, 4, P], F32, name="lg_5", tag="lg")
+        lg_5 = main.tile([P, 4, P], F32, name="lg_5", tag="lg", bufs=4)
         nc.scalar.activation(out=lg_5[:], in_=den_5[:], func=ACT.Abs_reciprocal_sqrt)
         lgs[STEPS - 3] = lg_5
+        log_den(STEPS - 2)
         exp_minus_log(STEPS - 3)
-        root_of_last_den(STEPS - 2)
         weigh(STEPS - 1, 0, 6)
-        root_of_last_den(STEPS - 1)
+        log_den(STEPS - 1)
+        exp_minus_log(STEPS - 2)
+        exp_minus_log(STEPS - 1)
+        for ob in range(4):
+            block_stats(STEPS - 4, ob)
+        first_part()
         divide(STEPS - 3)
-        moments(STEPS - 4, 1, 2)
-        moments(STEPS - 4, 3, 4)
 
-        tot = keep.tile([P, 2, 4], F32, name="tot")
-        dd = keep.tile([P, 4], F32, name="dd")
+        mean_var = keep.tile([P, 4, 2], F32, name="mean_var")
         gam_mean = keep.tile([P, 4], F32, name="gam_mean")
         rstd = keep.tile([P, 4], F32, name="rstd")
         gain = keep.tile([P, 4], F32, name="gain")
@@ -891,36 +890,17 @@ def tile_merge_pa_kernel(tc, x, w_c1, b_c1, w_q, w_k, w_v, bn_gamma, bn_beta, pr
         def col(t, ob):
             return t[:, ob:ob + 1]
 
-        part = {}
-
         def divide_block(s, ob):
             pump_to(("G", s, 6 * ob + 5))
-            if ob not in part:
-                once = main.tile([P, 4, ROW], F32, name="once", tag="once")
-                part[ob] = once
-            nc.vector.tensor_tensor(out=part[ob][:, end_rows(s), :], in0=nums[(s, ob)][:].rearrange("p (h f) -> p h f", h=2),
-                                    in1=lg_end[:, ob, end_rows(s), :], op=ALU.mult)
+            nc.vector.tensor_tensor(out=att_rows[:, ob, 7 - s:9 + s:2 * s + 1, :], in0=nums[(s, ob)][:].rearrange("p (h f) -> p h f", h=2),
+                                    in1=rds[s][:, ob, :].rearrange("p (h f) -> p h f", h=2), op=ALU.mult)
 
-        def last_sum(ob):
-            nc.vector.scalar_tensor_tensor(out=of_two_blocks(STEPS - 2, ob), in0=part[ob][:].rearrange("p (g r) f -> p g (r f)", g=2), scalar=1.0,
-                                           in1=lg_end[:, ob].rearrange("p (g r) f -> p g (r f)", g=2), op0=ALU.mult, op1=ALU.mult,
-                                           accum_out=msums[:, 0, ob, ENDS:ENDS + 1])
-
-        def last_squares(ob):
-            junk = main.tile([P, 2, P], F32, name="junk2", tag="junk2")
-            nc.scalar.activation(out=junk[:], in_=of_two_blocks(STEPS - 2, ob), func=ACT.Square, bias=col(neg_pivot, ob), scale=1.0,
-                                 accum_out=msums[:, 1, ob, ENDS:ENDS + 1])
-
-        def totals(ob):
-            nc.vector.tensor_reduce(out=tot[:, :, ob:ob + 1], in_=msums[:, :, ob:ob + 1, :], axis=mybir.AxisListType.X, op=ALU.add)
+        def mean_and_var(ob):
+            nc.vector.bn_aggr(out=mean_var[:, ob, :], in_=bn_parts[:, ob].rearrange("p g i -> p (g i)"))
 
         def statistics(ob):
-            nc.vector.scalar_tensor_tensor(out=col(dd, ob), in0=tot[:, 0, ob:ob + 1], scalar=1.0 / (NPIX * NPIX), in1=tot[:, 0, ob:ob + 1],
-                                           op0=ALU.mult, op1=ALU.mult)
-            nc.vector.tensor_scalar(out=col(gam_mean, ob), in0=tot[:, 0, ob:ob + 1], scalar1=col(gam_n, ob), scalar2=col(gam_pivot, ob),
-                                    op0=ALU.mult, op1=ALU.add)
-            nc.scalar.activation(out=col(rstd, ob), in_=tot[:, 1, ob:ob + 1], func=ACT.Abs_reciprocal_sqrt, bias=col(dd, ob),
-                                 scale=-1.0 / NPIX)
+            nc.vector.tensor_scalar(out=col(gam_mean, ob), in0=mean_var[:, ob, 0:1], scalar1=col(gam_p, ob), scalar2=None, op0=ALU.mult)
+            nc.scalar.activation(out=col(rstd, ob), in_=mean_var[:, ob, 1:2], func=ACT.Abs_reciprocal_sqrt, bias=BN_EPS, scale=1.0)
             nc.scalar.activation(out=col(gain, ob), in_=col(rstd, ob), func=ACT.Copy, scale=col(gam_f, ob))
             nc.scalar.activation(out=col(shift, ob), in_=col(rstd, ob), func=ACT.Identity, bias=col(neg_beta, ob),
                                  scale=col(gam_mean, ob))
@@ -974,48 +954,48 @@ def tile_merge_pa_kernel(tc, x, w_c1, b_c1, w_q, w_k, w_v, bn_gamma, bn_beta, pr
                                            op0=ALU.mult, op1=ALU.subtract)
             nc.sync.dma_start(out=out_v[:, ob, b0:b1], in_=res[:].rearrange("p (b f) -> p b f", b=NB)[:, b0:b1])
 
+        B5 = STEPS - 3
         B6 = STEPS - 2
         B7 = STEPS - 1
+        block_stats(B5, 0)
         divide_block(B6, 0)
-        divide_block(B7, 0)
+        block_stats(B5, 1)
         divide_block(B6, 1)
-        last_sum(0)
-        last_squares(0)
-        divide_block(B7, 1)
+        block_stats(B5, 2)
         divide_block(B6, 2)
-        last_sum(1)
-        moments(STEPS - 4, 5, 6)
-        last_squares(1)
+        block_stats(B5, 3)
+        nc.vector.tensor_copy(out=bn_parts[:, :, 0, 1:3], in_=first_four[:])
+        divide_block(B7, 0)
+        divide_block(B7, 1)
+        block_stats(B6, 0)
         divide_block(B7, 2)
-        totals(0)
-        divide_block(B6, 3)
+        mean_and_var(0)
+        block_stats(B6, 1)
         statistics(0)
         normalise(0)
-        last_sum(2)
-        moments(STEPS - 4, 7, 8)
-        last_squares(2)
+        minus_part(0)
+        divide_block(B6, 3)
+        mean_and_var(1)
         divide_block(B7, 3)
-        totals(1)
         normalise_on_vector(0)
-        minus_part_on_vector(0)
         statistics(1)
-        last_sum(3)
-        last_squares(3)
         normalise(1)
         minus_part(1)
-        totals(2)
+        block_stats(B6, 2)
+        block_stats(B6, 3)
+        mean_and_var(2)
         prelu_and_store(0)
         statistics(2)
-        normalise_on_vector(1)
-        totals(3)
         normalise(2)
         minus_part(2)
+        normalise_on_vector(1)
+        mean_and_var(3)
         prelu_and_store(1)
         statistics(3)
         normalise_on_vector(2)
         normalise(3)
         last_parts()
-        prelu_and_store(2)
         normalise_on_vector(3, 2, 4)
+        prelu_and_store(2)
         prelu_and_store(3, 0, 2)
         prelu_and_store(3, 2, 4)

@@ -901,7 +901,7 @@ def tile_merge_pa_kernel(tc, x, w_c1, b_c1, w_q, w_k, w_v, bn_gamma, bn_beta, pr
         def statistics(ob):
             nc.vector.tensor_scalar(out=col(gam_mean, ob), in0=mean_var[:, ob, 0:1], scalar1=col(gam_p, ob), scalar2=None, op0=ALU.mult)
             nc.scalar.activation(out=col(rstd, ob), in_=mean_var[:, ob, 1:2], func=ACT.Abs_reciprocal_sqrt, bias=BN_EPS, scale=1.0)
-            nc.scalar.activation(out=col(gain, ob), in_=col(rstd, ob), func=ACT.Copy, scale=col(gam_f, ob))
+            nc.scalar.activation(out=col(gain, ob), in_=col(rstd, ob), func=ACT.Identity, scale=col(gam_f, ob))
             nc.scalar.activation(out=col(shift, ob), in_=col(rstd, ob), func=ACT.Identity, bias=col(neg_beta, ob),
                                  scale=col(gam_mean, ob))
 
@@ -984,14 +984,14 @@ def tile_merge_pa_kernel(tc, x, w_c1, b_c1, w_q, w_k, w_v, bn_gamma, bn_beta, pr
         block_stats(B6, 2)
         block_stats(B6, 3)
         mean_and_var(2)
+        mean_and_var(3)
         prelu_and_store(0)
         statistics(2)
         normalise(2)
+        statistics(3)
         minus_part(2)
         normalise_on_vector(1)
-        mean_and_var(3)
         prelu_and_store(1)
-        statistics(3)
         normalise_on_vector(2)
         normalise(3)
         last_parts()

import math
from contextlib import ExitStack

import concourse.mybir as mybir
from concourse.masks import make_identity

F32 = mybir.dt.float32
BF16 = mybir.dt.bfloat16
I32 = mybir.dt.int32
U8 = mybir.dt.uint8
FP8X4 = mybir.dt.float8_e4m3fn_x4
ALU = mybir.AluOpType
ACT = mybir.ActivationFunctionType

P = 128
NB = 4
NPIX = 1024
ROW = 64
STEPS = 8
BN_EPS = 1e-5
BANK_DT = BF16
AHEAD = 3
SHARE_FROM = 0
IDLE_STEP_1 = 2
IDLE_HEAD = 2
WARM_UP = 4
EARLY_FROM = 1
FIRST_LENT = 2
LATE = 2
LAST_BANKS = (("k_ps", 3), ("k_ps", 3), ("k_ps", 3), ("v_ps", 3), ("v_ps", 3), ("v_ps", 3), ("den", 1), ("num", 1))
LAST_ON_VECTOR = 3
PIECES = ((0, 4), (4, 4), (8, 8))
HAAR_ON_VECTOR = ((0, 0), (0, 1), (1, 2), (1, 3), (2, 2))
TURNED = (0, 1)
FIRST_IN_HALVES = (0, 3)
W_C1, W_K, W_Q, W_V, W_KN = 0, 1, 2, 3, 4
INNER, OWN, OUTER = -1, 0, 1
WINDOWS = ((INNER, 0), (INNER, 2), (OWN, 0), (OWN, 2), (OUTER, 0), (OUTER, 2), (OUTER, 1))
SCORES = 7
OUTWARDS = 6
ITSELF = 7
INWARDS = 8
SHARED_FROM = 1
GROUPS = ((0, 2), (2, 5), (5, 7))
TWO_GROUPS = ((0, 2), (2, 7))
IN_TWO = (0, 1, 2, 3, 4, 5, 6)
CLIP = 32.0
LAST = STEPS - 1
Y_ROWS = 2 * (STEPS + 1)
LAST_WINDOWS = ((INNER, 0), (INNER, 1), (INNER, 2), (OWN, 0), (OWN, 2), (OWN, 1))
LAST_GROUPS = ((0, 4), (4, 6))
LAST_EXPS = (7, 0, 1, 2, 3, 4, 5)

FLOPS = 4 * 2 * 512 * 512 * 1024


def tile_merge_pa_kernel(tc, x, w_c1, b_c1, w_q, w_k, w_v, bn_gamma, bn_beta, prelu_a, out):
    nc = tc.nc
    with ExitStack() as ctx:
        keep = ctx.enter_context(tc.tile_pool(name="keep", bufs=1))
        mid = ctx.enter_context(tc.tile_pool(name="mid", bufs=1))
        main = ctx.enter_context(tc.tile_pool(name="main", bufs=2))
        psm = ctx.enter_context(tc.psum_pool(name="psm", bufs=1))
        ctx.enter_context(tc.manual_schedule())

        weights = (w_c1, w_k, w_q, w_v)
        w_all = main.tile([P, 4, 4, 512], BF16, name="w_all", tag="z", bufs=3, align_bytes=256)
        x_ab = main.tile([P, 2, NB, 4, 256], BF16, name="x_ab", tag="ev", bufs=2, align_bytes=256)
        x_c = main.tile([P, NB, 4, 512], BF16, name="x_c", tag="ev", bufs=2, align_bytes=256)

        def x_piece(pc, b):
            return x_c[:, b] if pc == 2 else x_ab[:, pc, b]

        def load_w(i, parts=1):
            n = 4 // parts
            for h in range(parts):
                nc.sync.dma_start(out=w_all[:, i, n * h:n * (h + 1)],
                                  in_=weights[i].rearrange("(c r) k -> c r k", r=4)[:, n * h:n * (h + 1)])

        def load_x(pc):
            row0, nr = PIECES[pc]
            for b in range(NB):
                rows = x[b].rearrange("(p j) (r a) w -> p j r (a w)", j=4, a=2)
                if pc == 0:
                    for j0, j1 in (((0, 2), (2, 4)) if b == FIRST_IN_HALVES[1] else ((0, 4),)):
                        nc.sync.dma_start(out=x_piece(pc, b)[:, j0:j1], in_=rows[:, j0:j1, 6:10].rearrange("p j r f -> p j (r f)"))
                else:
                    n = nr // 2
                    for h, r in enumerate((8 - row0 // 2 - n, 8 + row0 // 2)):
                        nc.sync.dma_start(out=x_piece(pc, b)[:, :, ROW * n * h:ROW * n * (h + 1)],
                                          in_=rows[:, :, r:r + n].rearrange("p j r f -> p j (r f)"))

        bias_bf = keep.tile([P, 4], BF16, name="bias_bf")
        load_w(W_C1)
        load_x(0)
        nc.scalar.dma_start(out=bias_bf[:], in_=b_c1.rearrange("(p t) -> p t", t=4))
        load_w(W_Q, 2)
        load_w(W_K, 2)
        load_x(1)
        load_w(W_V)
        load_x(2)

        ident = keep.tile([P, P], F32, name="ident", align_bytes=256)
        make_identity(nc, ident[:])
        ident_bf = keep.tile([P, P], BF16, name="ident_bf")
        make_identity(nc, ident_bf[:])
        to_ybx = keep.tile([P, P], F32, name="to_ybx", align_bytes=256)
        nc.gpsimd.tensor_copy(out=to_ybx[:].rearrange("p (y b x) -> p y b x", b=NB, x=16),
                              in_=ident[:].rearrange("p (y x b) -> p y b x", b=NB, x=16))

        gam_bf = keep.tile([P, 4], BF16, name="gam_bf")
        bet_bf = keep.tile([P, 4], BF16, name="bet_bf")
        a_bf = keep.tile([P, 1], BF16, name="a_bf")

        warm = keep.tile([P, 1], F32, name="warm")
        nc.scalar.activation(out=warm[:], in_=ident[:, 0:1], func=ACT.Exp)

        w_codes = []
        w_scales = []
        for i in range(5):
            wct = keep.tile([P, 512], I32, name="w_codes%d" % i, align_bytes=256)
            wst = keep.tile([P, 512], U8, name="w_scales%d" % i, align_bytes=256)
            w_codes.append(wct)
            w_scales.append(wst)
        nc.vector.memset(w_codes[W_KN][:], 0)
        nc.vector.memset(w_scales[W_KN][:].bitcast(I32), 0)
        ll_codes = keep.tile([P, NPIX], I32, name="ll_codes", align_bytes=64)
        ll_scales = keep.tile([P, NPIX], U8, name="ll_scales", align_bytes=64)
        y_codes = []
        y_scales = []
        for d in range(3):
            yct = keep.tile([P, Y_ROWS * ROW], I32, name="y_codes%d" % d, align_bytes=256)
            yst = keep.tile([P, Y_ROWS * ROW], U8, name="y_scales%d" % d, align_bytes=256)
            if d != 1:
                nc.gpsimd.memset(yct[:].bitcast(F32), 0.0)
            nc.gpsimd.memset(yst[:].bitcast(F32), 0.0)
            y_codes.append(yct)
            y_scales.append(yst)

        att = keep.tile([P, 4, NPIX], F32, name="att")
        msums = keep.tile([P, 2, 4, 2], F32, name="msums")
        bn_parts = keep.tile([P, 4, 7, 3], F32, name="bn_parts")
        first_four = keep.tile([P, 4, 2], F32, name="first_four")
        nc.vector.memset(bn_parts[:, :, 0, 0], 4.0 * P)
        neg_pivot = keep.tile([P, 4], F32, name="neg_pivot")
        one_minus_a = keep.tile([P, 1], F32, name="one_minus_a")
        gam_f = keep.tile([P, 4], F32, name="gam_f")
        gam_p = keep.tile([P, 4], F32, name="gam_p")
        neg_beta = keep.tile([P, 4], F32, name="neg_beta")
        bias_full = keep.tile([P, ROW, 4], BF16, name="bias_full")

        ll = mid.tile([P, NPIX, 4], BF16, name="ll", align_bytes=64)
        y_mid = mid.tile([P, NPIX, 4], BF16, name="y_mid", align_bytes=64)
        ll_by_image = ll[:].rearrange("p (y b x) j -> p b y x j", b=NB, x=16)
        ll_flat = ll[:].rearrange("p c j -> p (c j)")
        nc.sync.dma_start(out=gam_bf[:], in_=bn_gamma.rearrange("(p t) -> p t", t=4))
        nc.sync.dma_start(out=bet_bf[:], in_=bn_beta.rearrange("(p t) -> p t", t=4))
        nc.sync.dma_start(out=a_bf[:], in_=prelu_a.partition_broadcast(P))

        haar_sum = keep.tile([P, 32], BF16, name="haar_sum")
        with nc.allow_low_precision(reason="every sum is a single one"):
            nc.vector.tensor_reduce(out=haar_sum[:].rearrange("p (i x) -> p i x", i=2),
                                    in_=ident_bf[:].rearrange("p (i a x e) -> p i x a e", i=2, a=2, x=16), axis=mybir.AxisListType.XY,
                                    op=ALU.add)
        x_turned = {}
        zs = {}
        ws = {}
        evs = {}
        nums = {}
        dens = {}
        q_sbs = {}
        rds = {}
        lgs = {}
        ms = {}
        banks = {}
        ev_sums = []

        def ok(s):
            return 0 <= s < STEPS

        def window(dst, place, d, wi, start=True, stop=True, channels=slice(0, 512)):
            c0 = P * (place + 1)
            nc.tensor.matmul_mx(out=dst, lhsT=y_codes[d][:, c0:c0 + P].bitcast(FP8X4),
                                lhsT_scale=y_scales[d][:, c0:c0 + P],
                                rhs=w_codes[wi][:, channels].bitcast(FP8X4), rhs_scale=w_scales[wi][:, channels],
                                start=start, stop=stop)

        def first_conv(bank, r):
            cols = slice(P * r, P * (r + 1))
            for t in range(4):
                nc.tensor.matmul_mx(out=bank[:, t, :],
                                    lhsT=w_codes[W_C1][:, P * t:P * (t + 1)].bitcast(FP8X4),
                                    lhsT_scale=w_scales[W_C1][:, P * t:P * (t + 1)],
                                    rhs=ll_codes[:, cols].bitcast(FP8X4), rhs_scale=ll_scales[:, cols],
                                    start=True, stop=True)

        def add_up(dst, src, i):
            ob = i // 9
            j = i % 9
            nc.tensor.matmul(out=dst[:, ob, :], lhsT=src(j)[:, P * ob:P * (ob + 1)], rhs=to_ybx[:],
                             is_transpose=True, start=(j == 0), stop=(j == 8))

        def last_bank(s, ob):
            tag, bufs = LAST_BANKS[2 * ob + s - (STEPS - 2)]
            bank = psm.tile([P, P], F32, name="num_end", tag=tag, bufs=bufs)
            nums[(s, ob)] = bank

        def emit_pe(tok):
            kind, s, j = tok
            if kind == "q":
                q_ps = psm.tile([P, 512], F32, name="q_ps", tag="k_ps", bufs=3)
                window(q_ps[:], s, 1, W_Q)
                banks[tok] = q_ps
            elif kind == "b":
                half_bank = psm.tile([P, 256], F32, name="k_half", tag=("k_ps" if j == 0 else ("num", "den")[s]), bufs=(3 if j == 0 else 1))
                window(half_bank[:], (OUTER, OWN)[s], 1, W_K, True, False, slice(256 * j, 256 * (j + 1)))
                banks[tok] = half_bank
            elif kind == "B":
                window(banks[("b", s, j)][:], (OWN, INNER)[s], 1, W_KN, False, True, slice(256 * j, 256 * (j + 1)))
            elif kind == "k":
                if s >= FIRST_LENT and j == bank_order(s)[AHEAD]:
                    k_ps = psm.tile([P, 512], F32, name="k_lent", tag="den", bufs=1)
                else:
                    k_ps = psm.tile([P, 512], F32, name="k_ps", tag="k_ps", bufs=3)
                if s == LAST:
                    window(k_ps[:], s + LAST_WINDOWS[j][0], LAST_WINDOWS[j][1], W_K)
                elif j == INWARDS:
                    window(k_ps[:], s, 1, W_K, True, False)
                    window(k_ps[:], s + INNER, 1, W_KN, False, True)
                else:
                    window(k_ps[:], s + WINDOWS[j][0], WINDOWS[j][1], W_K, True, False)
                    window(k_ps[:], s, 1, W_KN, False, True)
                banks[tok] = k_ps
            elif kind == "d":
                if j == 0:
                    idle = psm.tile([P, 512], F32, name="idle", tag="num", bufs=1)
                    banks["idle"] = idle
                nc.tensor.matmul_mx(out=banks["idle"][:], lhsT=w_codes[W_KN][:, 0:P].bitcast(FP8X4), lhsT_scale=w_scales[W_KN][:, 0:P],
                                    rhs=w_codes[W_KN][:].bitcast(FP8X4), rhs_scale=w_scales[W_KN][:], start=True, stop=True)
            elif kind in ("v", "u", "o"):
                if tok in in_k_banks:
                    v_ps = psm.tile([P, 512], F32, name="v_in_k", tag="k_ps", bufs=3)
                elif tok in lent_to_v:
                    v_ps = psm.tile([P, 512], F32, name="v_lent", tag="num", bufs=1)
                else:
                    v_ps = psm.tile([P, 512], F32, name="v_ps", tag="v_ps", bufs=3)
                window(v_ps[:], s, j, W_V)
                banks[tok] = v_ps
            elif kind == "c":
                if s == STEPS - 1:
                    bank = psm.tile([P, 4, P], BANK_DT, name="bank_last", tag="num", bufs=1)
                else:
                    bank = psm.tile([P, 4, P], BANK_DT, name="bank", tag="v_ps", bufs=3)
                first_conv(bank, s)
                banks[tok] = bank
            elif kind == "C":
                c0 = ROW * PIECES[s][0]
                n = ROW * PIECES[s][1]
                if j == 3:
                    wide = psm.tile([P, n], BANK_DT, name="wide_last", tag="num", bufs=1)
                else:
                    wide = psm.tile([P, n], BANK_DT, name="wide", tag="v_ps", bufs=3)
                nc.tensor.matmul_mx(out=wide[:], lhsT=w_codes[W_C1][:, P * j:P * (j + 1)].bitcast(FP8X4),
                                    lhsT_scale=w_scales[W_C1][:, P * j:P * (j + 1)],
                                    rhs=ll_codes[:, c0:c0 + n].bitcast(FP8X4), rhs_scale=ll_scales[:, c0:c0 + n],
                                    start=True, stop=True)
                banks[tok] = wide
            elif kind == "w":
                words = w_all[:, s].bitcast(F32)
                wT = psm.tile([P, 2, 2, P], F32, name="wT", tag=("k_ps" if s != W_V else "v_ps"), bufs=3)
                for rr in range(2):
                    for u in range(2):
                        nc.tensor.transpose(wT[:, rr, u, :], words[:, 2 * j + rr, u:256:2], ident[:])
                banks[tok] = wT
            elif kind in ("h", "i"):
                nr = PIECES[s][1]
                taps = x_piece(s, j).rearrange("p j (i a x e) -> p j i a x e", a=2, x=16, e=2)
                if j == NB - 1 and kind == "h":
                    hs = psm.tile([P, 512], F32, name="hs_last", tag="den", bufs=1)
                else:
                    hs = psm.tile([P, 512], F32, name="hs", tag="v_ps", bufs=3)
                j0 = 2 if kind == "i" else 0
                nj = 2 if s == 2 or (s, j) == FIRST_IN_HALVES else 4
                for n in range(4):
                    nc.tensor.matmul(out=hs[:, 0:16 * nj * nr].rearrange("p (j i x) -> p j i x", j=nj, x=16), lhsT=ident_bf[:],
                                     rhs=taps[:, j0:j0 + nj, :, n // 2, :, n % 2], start=(n == 0), stop=(n == 3))
                banks[tok] = hs
            elif kind == "T":
                xt = psm.tile([P, 8, P], BF16, name="xt", tag="v_ps", bufs=3)
                for i in range(8):
                    nc.tensor.transpose(xt[:, i, :], x_c[:, s, 2 * j + i // 4, P * (i % 4):P * (i % 4 + 1)], ident_bf[:])
                banks[tok] = xt
            elif kind == "H":
                if s == NB - 1:
                    hs = banks[("h", 2, s)]
                else:
                    hs = psm.tile([P, 512], F32, name="hs_turned", tag="v_ps", bufs=3)
                for i in range(8 if s == NB - 1 else 0, 16):
                    nc.tensor.matmul(out=hs[:, 32 * i:32 * (i + 1)], lhsT=x_turned[s][:, i, :], rhs=haar_sum[:], start=True, stop=True)
                banks[tok] = hs
            elif kind == "F":
                if j == 0:
                    if s == STEPS - 1:
                        den = psm.tile([P, 4, P], F32, name="den_last", tag="v_ps", bufs=3)
                    else:
                        den = psm.tile([P, 4, P], F32, name="den", tag="den", bufs=1)
                    dens[s] = den
                if s == LAST:
                    n = len(LAST_EXPS)
                    nc.tensor.matmul(out=dens[s][:, j // n, :], lhsT=zs[s][:, LAST_EXPS[j % n], P * (j // n):P * (j // n + 1)],
                                     rhs=to_ybx[:], is_transpose=True, start=(j % n == 0), stop=(j % n == n - 1))
                else:
                    add_up(dens[s], lambda i: exp_of(s, i), j)
            elif kind == "G" and s == STEPS - 2:
                ob = j // 6
                if j % 6 == 0:
                    last_bank(s, ob)
                term = ev_sums[0][:, j % 6, :] if j % 6 < 3 else evs[s][:, 3 + j % 6, :]
                nc.tensor.matmul(out=nums[(s, ob)][:], lhsT=term[:, P * ob:P * (ob + 1)], rhs=to_ybx[:],
                                 is_transpose=True, start=(j % 6 == 0), stop=(j % 6 == 5))
            elif kind == "G" and s == STEPS - 1:
                ob = j // 6
                if j % 6 == 0:
                    last_bank(s, ob)
                nc.tensor.matmul(out=nums[(s, ob)][:], lhsT=evs[s][:, j % 6, P * ob:P * (ob + 1)], rhs=to_ybx[:],
                                 is_transpose=True, start=(j % 6 == 0), stop=(j % 6 == 5))
            else:
                if j == 0:
                    num = psm.tile([P, 4, P], F32, name="num", tag="num", bufs=1)
                    nums[s] = num
                add_up(nums[s], lambda i: evs[s][:, i, :], j)

        def exp_of(s, slot):
            return ws[s][:] if slot == INWARDS else zs[s][:, slot, :]

        def bank_order(s):
            if s == LAST:
                return tuple(range(len(LAST_WINDOWS)))
            if s == 0:
                return (OUTWARDS, INWARDS, 0, 1, 2, 3, 4, 5)
            if s <= SHARED_FROM:
                return (0, 1, 2, 3, INWARDS, 4, 5, OUTWARDS)
            return (0, 1, 2, 3, 4, 5, OUTWARDS)

        def products(a):
            todo = []
            if a == LAST:
                return [(("v" if place == OWN else "u", a + place, d), a, j) for j, (place, d) in enumerate(LAST_WINDOWS)]
            if a <= SHARE_FROM:
                todo.extend([(("u", a - 1, d), a, slot) for d, slot in ((0, 0), (2, 1), (1, INWARDS))])
            outer = [(("o", a + 1, d), a, slot) for d, slot in ((0, 4), (2, 5), (1, OUTWARDS))]
            own = []
            for d, slot, inner_slot in ((0, 2, 0), (2, 3, 1), (1, ITSELF, INWARDS)):
                own.append((("v", a, d), a, slot))
                if a + 1 < LAST and a >= SHARE_FROM:
                    own.append((("v", a, d), a + 1, inner_slot))
            if a == STEPS - 2:
                return todo + outer[:2] + own[:2] + outer[2:] + own[2:]
            return todo + outer + own

        def v_banks(a):
            toks = []
            for tok, s, slot in products(a):
                if tok not in toks:
                    toks.append(tok)
            return toks

        lent_to_v = [v_banks(a)[3] for a in range(STEPS - 3)]
        in_k_banks = v_banks(STEPS - 3)[3:] + v_banks(STEPS - 2)[3:] + v_banks(STEPS - 1)[3:]

        def scores_of(s):
            return len(bank_order(s))

        def den_terms(s):
            return 4 * len(LAST_EXPS) if s == LAST else 36

        def on_pe(pc):
            toks = [("h", pc, b) for b in range(NB) if (pc, b) not in HAAR_ON_VECTOR and (pc < 2 or b not in TURNED)]
            return toks + [("i", 0, FIRST_IN_HALVES[1])] if pc == FIRST_IN_HALVES[0] else toks

        pe_list = [("d", 0, i) for i in range(WARM_UP)] + [("w", W_C1, 0), ("w", W_C1, 1)] + [("d", 3, i) for i in range(IDLE_HEAD)] + on_pe(0) + [("w", W_Q, 0), ("w", W_Q, 1), ("c", 0, 0), ("c", 1, 0),
                                                                 ("w", W_K, 0), ("w", W_K, 1)] + on_pe(1)
        pe_list += [("q", 0, 0)] + [("b", 0, 0), ("B", 0, 0), ("b", 1, 0), ("B", 1, 0), ("b", 0, 1), ("b", 1, 1), ("B", 0, 1), ("B", 1, 1)]
        pe_list += [("k", 0, j) for j in bank_order(0)[2:AHEAD]]
        for s in range(STEPS + 2):
            a = s - 2
            if ok(s):
                pe_list.extend([("k", s, j) for j in bank_order(s)[AHEAD if s == 0 else AHEAD + LATE:]])
            if ok(s + 1):
                pe_list.append(("q", s + 1, 0))
            if s == 0:
                pe_list.extend([("w", W_V, 0), ("w", W_V, 1)] + [("C", 1, t) for t in range(4)] + [("T", 0, 0), ("T", 0, 1), ("T", 1, 0)] + on_pe(2))
            if s == 1:
                pe_list.extend([("T", 1, 1), ("H", 0, 0), ("T", 3, 1), ("H", 1, 0), ("H", 3, 0)])
                pe_list.extend([("k", s + 1, j) for j in bank_order(s + 1)[:AHEAD]] + [("d", 1, i) for i in range(IDLE_STEP_1)] + [("C", 2, t) for t in range(4)])
            vb = v_banks(a)[3 if a >= EARLY_FROM else 0:] if ok(a) else []
            early = v_banks(a + 1)[:3] if ok(a + 1) and a + 1 >= EARLY_FROM else []
            den_sums = [("F", a, i) for i in range(den_terms(a))] if ok(a) else []
            num_sums = [("G", a, i) for i in range(36)] if ok(a) and a < STEPS - 2 else []
            if a == STEPS - 2:
                pe_list.extend(vb + den_sums)
                vb = []
                den_sums = []
            if a == STEPS - 1:
                pe_list.extend(vb)
                vb = []
            if s == STEPS - 1:
                pe_list.extend(den_sums[:9] + vb + den_sums[9:])
                vb = []
                den_sums = []
            if ok(a) and a < EARLY_FROM:
                pe_list.extend(vb[:3] + den_sums[:9] + vb[3:7] + den_sums[9:18] + vb[7:])
            else:
                pe_list.extend(den_sums[:18] + vb)
            if ok(s + 1) and s != 1:
                pe_list.extend([("k", s + 1, j) for j in bank_order(s + 1)[:AHEAD]])
            pe_list.extend(den_sums[18:])
            pe_list.extend(num_sums)
            late_k = [("k", s + 1, j) for j in bank_order(s + 1)[AHEAD:AHEAD + LATE]] if ok(s + 1) else []
            pe_list.extend(late_k[:1] + early + late_k[1:])
        for ob in range(4):
            pe_list.extend([("G", STEPS - 2, 6 * ob + j) for j in range(6)])
            pe_list.extend([("G", STEPS - 1, 6 * ob + j) for j in range(6)])

        done = set()
        pos = [0]

        def pump_to(tok):
            while tok not in done:
                nxt = pe_list[pos[0]]
                pos[0] += 1
                emit_pe(nxt)
                done.add(nxt)

        def weight_copies(i):
            grouped = main.tile([P, 2048], BF16, name="grouped", tag="grouped", bufs=2, align_bytes=64)
            gwords = grouped[:].bitcast(F32).rearrange("p (r c u) -> p r c u", r=4, u=2)
            for h in range(2):
                pump_to(("w", i, h))
                nc.scalar.copy(out=gwords[:, 2 * h:2 * h + 2], in_=banks[("w", i, h)][:].rearrange("p r u c -> p r c u"))
            return grouped

        def quant_w(i, grouped):
            nc.vector.quantize_mx(out=w_codes[i][:].bitcast(FP8X4), scales=w_scales[i][:], in_=grouped[:])

        def quant_w_half(i, grouped, h):
            nc.vector.quantize_mx(out=w_codes[i][:, 256 * h:256 * (h + 1)].bitcast(FP8X4), scales=w_scales[i][:, 256 * h:256 * (h + 1)],
                                  in_=grouped[:, 1024 * h:1024 * (h + 1)])

        def halve(pc, b, sums, j0=0, j1=4):
            row0, nr = PIECES[pc]
            nc.scalar.activation(out=ll_by_image[:, b, row0:row0 + nr, :, j0:j1],
                                 in_=sums.rearrange("p (j y x) -> p y x j", j=j1 - j0, x=16),
                                 func=ACT.Copy, scale=0.5)

        def haar_from_pe(pc):
            for tok in on_pe(pc):
                pump_to(tok)
                n = 2 * 16 * PIECES[pc][1]
                if tok[0] == "i":
                    nc.vector.tensor_scalar(out=ll_by_image[:, tok[2], 0:PIECES[pc][1], :, 2:4],
                                            in0=banks[tok][:, 0:n].rearrange("p (j y x) -> p y x j", j=2, x=16), scalar1=0.5, scalar2=None,
                                            op0=ALU.mult)
                elif tok[1:] == FIRST_IN_HALVES:
                    halve(pc, tok[2], banks[tok][:, 0:n], 0, 2)
                else:
                    halve(pc, tok[2], banks[tok][:, 0:2 * n])

        def haar_on_vector(pc, images, on_gpsimd=False, between=None):
            eng = nc.gpsimd if on_gpsimd else nc.vector
            nr = PIECES[pc][1]
            row_sums = []
            for b in images:
                if on_gpsimd:
                    s1 = main.tile([P, 4, nr, 32], F32, name="s1_late", tag="grouped", bufs=2, align_bytes=64)
                    row_sums.append(s1)
                else:
                    s1 = main.tile([P, 4, nr, 32], F32, name="s1", tag="s1", bufs=2)
                    row_sums.append(s1)
            for b, s1 in zip(images, row_sums):
                rows = x_piece(pc, b).rearrange("p j (i a w) -> p j i a w", a=2, w=32)
                eng.tensor_tensor(out=s1[:], in0=rows[:, :, :, 0, :], in1=rows[:, :, :, 1, :], op=ALU.add)
            sums = []
            for b, s1 in zip(images, row_sums):
                pairs = s1[:].rearrange("p j i (x e) -> p (j i x) e", e=2)
                s2 = main.tile([P, ROW * nr], F32, name="s2", tag="s2", bufs=3)
                if between is not None and b == images[-1]:
                    between()
                eng.tensor_tensor(out=s2[:], in0=pairs[:, :, 0], in1=pairs[:, :, 1], op=ALU.add)
                if between is None:
                    halve(pc, b, s2[:])
                sums.append((b, s2))
            return sums

        def haar_by_reduce(pc, b):
            nr = PIECES[pc][1]
            taps = x_piece(pc, b).rearrange("p j (i a x e) -> p j i x a e", a=2, x=16, e=2)
            s2 = main.tile([P, ROW * nr], F32, name="s2_red", tag="s2", bufs=3)
            nc.vector.tensor_reduce(out=s2[:].rearrange("p (j i x) -> p j i x", j=4, x=16), in_=taps, axis=mybir.AxisListType.XY, op=ALU.add)
            return s2

        def turn_copies(b, halves):
            if b not in x_turned:
                turned = main.tile([P, 16, P], BF16, name="turned", tag="s1", bufs=2)
                x_turned[b] = turned
            for h in halves:
                pump_to(("T", b, h))
                nc.scalar.copy(out=x_turned[b][:, 8 * h:8 * (h + 1)].rearrange("p i c -> p (i c)").bitcast(F32),
                               in_=banks[("T", b, h)][:].rearrange("p i c -> p (i c)").bitcast(F32))

        def haar_from_turned(b, j0=0):
            pump_to(("H", b, 0))
            halve(2, b, banks[("H", b, 0)][:, P * j0:512], j0)

        def quant_ll(pc):
            c0 = ROW * PIECES[pc][0]
            n = ROW * PIECES[pc][1]
            nc.vector.quantize_mx(out=ll_codes[:, c0:c0 + n].bitcast(FP8X4), scales=ll_scales[:, c0:c0 + n],
                                  in_=ll_flat[:, 4 * c0:4 * (c0 + n)])

        def add_bias(r):
            pump_to(("c", r, 0))
            for yy in range(2):
                c0 = ROW * (2, 0, 1, 3)[2 * r + yy]
                nc.vector.tensor_tensor(out=y_mid[:, c0:c0 + ROW, :].rearrange("p (x b) t -> p x b t", b=NB),
                                        in0=banks[("c", r, 0)][:, :, ROW * yy:ROW * (yy + 1)].rearrange("p t (b x) -> p x b t", b=NB),
                                        in1=bias_full[:].rearrange("p (x b) t -> p x b t", b=NB), op=ALU.add)

        def add_bias_on_scalar(pc):
            c0 = ROW * PIECES[pc][0]
            n = ROW * PIECES[pc][1]
            by_slot = main.tile([P, 4, n], BF16, name="by_slot", tag="by_slot", bufs=1)
            for t in range(4):
                pump_to(("C", pc, t))
                to = by_slot[:, t, :].rearrange("p (i h x b) -> p h i x b", h=2, x=16, b=NB)
                rows = banks[("C", pc, t)][:].rearrange("p (h i b x) -> p h i x b", h=2, x=16, b=NB)
                for h, half in enumerate((rows[:, 0, ::-1], rows[:, 1])):
                    nc.scalar.activation(out=to[:, h], in_=half, func=ACT.Identity, bias=bias_bf[:, t:t + 1], scale=1.0)
            return lambda: nc.scalar.copy(out=y_mid[:, c0:c0 + n, :], in_=by_slot[:].rearrange("p t n -> p n t"))

        def quant_y(pc):
            p0 = ROW * PIECES[pc][0]
            n = ROW * PIECES[pc][1]
            nc.vector.quantize_mx(out=y_codes[1][:, P + p0:P + p0 + n].bitcast(FP8X4),
                                  scales=y_scales[1][:, P + p0:P + p0 + n],
                                  in_=y_mid[:].rearrange("p c j -> p (c j)")[:, 4 * p0:4 * (p0 + n)])

        code_rows = [t[:].rearrange("p (r c) -> p r c", c=ROW) for t in y_codes]
        scale_rows = [t[:].bitcast(I32).rearrange("p (r c) -> p r c", c=ROW // 4) for t in y_scales]

        def turn_middle():
            for rows in (code_rows[1], scale_rows[1]):
                nc.vector.tensor_copy(out=rows[:, 0:2, :], in_=rows[:, 3:1:-1, :])

        def move_y(pc):
            r0 = 2 + PIECES[pc][0] if pc > 0 else 0
            r1 = 2 + PIECES[pc][0] + PIECES[pc][1]
            w = ROW // 4
            nc.vector.tensor_copy(out=code_rows[0][:, r0:r1, NB:ROW], in_=code_rows[1][:, r0:r1, 0:ROW - NB])
            nc.vector.tensor_copy(out=code_rows[2][:, r0:r1, 0:ROW - NB], in_=code_rows[1][:, r0:r1, NB:ROW])
            nc.vector.tensor_copy(out=scale_rows[0][:, r0:r1, 1:w], in_=scale_rows[1][:, r0:r1, 0:w - 1])
            nc.vector.tensor_copy(out=scale_rows[2][:, r0:r1, 0:w - 1], in_=scale_rows[1][:, r0:r1, 1:w])

        def q_copy(s):
            pump_to(("q", s, 0))
            q_sb = main.tile([P, 512], F32, name="q_sb", tag="q_sb")
            nc.scalar.copy(out=q_sb[:], in_=banks[("q", s, 0)][:])
            q_sbs[s] = q_sb

        def new_scores(s):
            z = main.tile([P, 8, 512], F32, name="z", tag="z", bufs=3, align_bytes=256)
            zs[s] = z

        def new_inwards(s):
            w = main.tile([P, 512], F32, name="w", tag="w", bufs=4, align_bytes=256)
            ws[s] = w

        def first_scores():
            new_scores(0)
            new_inwards(0)
            for h in range(2):
                for i in range(2):
                    pump_to(("B", i, h))
                    c = slice(256 * h, 256 * (h + 1))
                    nc.vector.tensor_tensor(out=exp_of(0, bank_order(0)[i])[:, c], in0=q_sbs[0][:, c], in1=banks[("b", i, h)][:], op=ALU.mult)

        def scores(s, i0, i1):
            for i in range(i0, i1):
                j = bank_order(s)[i]
                pump_to(("k", s, j))
                if i == 0:
                    new_scores(s)
                if j == INWARDS:
                    new_inwards(s)
                nc.vector.tensor_tensor(out=exp_of(s, j), in0=q_sbs[s][:], in1=banks[("k", s, j)][:], op=ALU.mult)

        def scores_inwards(s):
            new_inwards(s + 1)
            nc.vector.tensor_tensor(out=ws[s + 1][:], in0=q_sbs[s + 1][:], in1=banks[("k", s, OUTWARDS)][:], op=ALU.mult)

        def groups_of(s):
            return LAST_GROUPS if s == LAST else TWO_GROUPS if s in IN_TWO else GROUPS

        def subtract(s, g, eng):
            g0, g1 = groups_of(s)[g]
            z = zs[s]
            eng.tensor_tensor(out=z[:, g0:g1, :], in0=z[:, g0:g1, :], in1=ms[s][:].unsqueeze(1).to_broadcast([P, g1 - g0, 512]),
                              op=ALU.subtract)

        def tree_in_halves(s, between, on_vector=0, within=None, behind=None):
            z = zs[s]
            halves = (slice(0, 256), slice(256, 512))
            t1 = main.tile([P, 3, 512], F32, name="t1", tag="t1", bufs=1)
            n = 2 if s == LAST else 3
            for c in halves:
                nc.vector.tensor_tensor(out=t1[:, 0:n, c], in0=z[:, 0:n, c], in1=z[:, 6 - n:6, c] if s == LAST else z[:, 3:6, c], op=ALU.max)
            between()
            t2 = main.tile([P, 2, 512], F32, name="t2", tag="t2", bufs=1)
            for c in halves:
                nc.vector.tensor_tensor(out=t2[:, 0, c], in0=t1[:, 0, c], in1=t1[:, 1, c], op=ALU.max)
                if c == halves[0]:
                    if within is not None:
                        within()
                    if s < LAST:
                        nc.vector.tensor_tensor(out=t2[:, 1, :], in0=t1[:, 2, :], in1=z[:, 6, :], op=ALU.max)
            m = main.tile([P, 512], F32, name="m", tag="m")
            for c in halves:
                other = z[:, 2, c] if s == LAST else t2[:, 1, c]
                nc.vector.scalar_tensor_tensor(out=m[:, c], in0=t2[:, 0, c], scalar=0.0, in1=other, op0=ALU.max, op1=ALU.max)
            ms[s] = m
            if behind is not None:
                behind()
            for g in range(len(groups_of(s))):
                if 3 * g < on_vector:
                    subtract(s, g, nc.vector)
                elif on_vector == 0:
                    subtract(s, g, nc.gpsimd)
                if g == 0 and s < LAST:
                    nc.gpsimd.tensor_tensor(out=ws[s][:], in0=ws[s][:], in1=m[:], op=ALU.add)

        def exps(s, g):
            z = zs[s]
            if g == 0:
                if s == LAST:
                    nc.scalar.activation(out=z[:, ITSELF, :], in_=ms[s][:], func=ACT.Exp, scale=-1.0, bias=math.log(3.0))
                else:
                    nc.scalar.activation(out=z[:, ITSELF, :], in_=ms[s][:], func=ACT.Exp, scale=-1.0)
            g0, g1 = groups_of(s)[g]
            if s == LAST and g == 0:
                g1 -= 1
                nc.scalar.activation(out=z[:, g1, :], in_=z[:, g1, :], func=ACT.Relu, scale=-1.0, bias=CLIP)
                nc.scalar.activation(out=z[:, g0:g1, :], in_=z[:, g0:g1, :], func=ACT.Exp)
                nc.scalar.activation(out=z[:, g1, :], in_=z[:, g1, :], func=ACT.Exp, scale=-1.0, bias=CLIP)
            else:
                nc.scalar.activation(out=z[:, g0:g1, :], in_=z[:, g0:g1, :], func=ACT.Exp)
            if g == 0 and s + 1 < 4:
                q_copy(s + 2)
            if g == 0 and s < LAST:
                w = ws[s]
                nc.scalar.activation(out=w[:], in_=w[:], func=ACT.Relu, scale=1.0, bias=CLIP)
                nc.scalar.activation(out=w[:], in_=w[:], func=ACT.Exp, scale=-1.0, bias=CLIP)

        def weigh(a, i0, i1):
            for tok, s, slot in products(a)[i0:i1]:
                pump_to(tok)
                if s not in evs:
                    ev = main.tile([P, 9, 512], F32, name="ev", tag="ev", bufs=2, align_bytes=256)
                    evs[s] = ev
                nc.vector.tensor_tensor(out=evs[s][:, slot, :], in0=exp_of(s, slot), in1=banks[tok][:], op=ALU.mult)

        def log_den(s):
            pump_to(("F", s, den_terms(s) - 1))
            lg = main.tile([P, 4, P], F32, name="lg", tag="lg", bufs=4)
            nc.scalar.activation(out=lg[:], in_=dens[s][:], func=ACT.Abs_reciprocal_sqrt)
            lgs[s] = lg

        def exp_minus_log(s):
            rd = main.tile([P, 4, P], F32, name="rd", tag="rd", bufs=3)
            nc.scalar.activation(out=rd[:], in_=lgs[s][:], func=ACT.Square)
            rds[s] = rd

        def one_over_den(s):
            log_den(s)
            exp_minus_log(s)

        att_rows = att[:].rearrange("p o (y f) -> p o y f", f=ROW)
        att_pairs = att[:].rearrange("p o (g n) -> p o g n", n=P)

        def by_row(t):
            return t.rearrange("p o (h f) -> p o h f", h=2)

        def of_two_blocks(s, ob):
            i = s // 2
            return att_pairs[:, ob, 3 - i:5 + i:2 * i + 1, :]

        def divide(s, on_vector=4):
            pump_to(("G", s, 35))
            att_s = att_rows[:, :, 7 - s:9 + s:2 * s + 1, :]
            if on_vector < 4:
                num_sb = main.tile([P, 4 - on_vector, P], F32, name="num_sb", tag="num_sb")
                nc.scalar.copy(out=num_sb[:], in_=nums[s][:, on_vector:4, :])
            nc.vector.tensor_tensor(out=att_s[:, 0:on_vector], in0=by_row(nums[s][:, 0:on_vector, :]), in1=by_row(rds[s][:, 0:on_vector, :]),
                                    op=ALU.mult)
            if on_vector < 4:
                nc.gpsimd.tensor_tensor(out=att_s[:, on_vector:4], in0=by_row(num_sb[:]), in1=by_row(rds[s][:, on_vector:4, :]), op=ALU.mult)

        def block_stats(s, ob):
            i = 1 + 2 * (s - 4)
            nc.vector.bn_stats(out=bn_parts[:, ob, i:i + 2, :].rearrange("p g i -> p (g i)"),
                               in_=of_two_blocks(s, ob) if s == STEPS - 2 else att_rows[:, ob, 7 - s:9 + s:2 * s + 1, :])

        def first_part():
            half = keep.tile([P, 2, 4], F32, name="half")
            mean = keep.tile([P, 4], F32, name="mean")
            squared = keep.tile([P, 4], F32, name="squared")
            nc.gpsimd.tensor_tensor(out=half[:], in0=msums[:, :, :, 0], in1=msums[:, :, :, 1], op=ALU.add)
            nc.gpsimd.tensor_scalar(out=mean[:], in0=half[:, 0, :], scalar1=0.25 / P, scalar2=0.0, op0=ALU.mult, op1=ALU.add)
            nc.gpsimd.tensor_tensor(out=squared[:], in0=half[:, 0, :], in1=mean[:], op=ALU.mult)
            nc.gpsimd.tensor_tensor(out=first_four[:, :, 0], in0=mean[:], in1=neg_pivot[:], op=ALU.subtract)
            nc.gpsimd.tensor_tensor(out=first_four[:, :, 1], in0=half[:, 1, :], in1=squared[:], op=ALU.subtract)

        def moments(s, first=0, end=8):
            for i in range(first, end):
                ob = i // 2
                kind = i % 2
                junk = main.tile([P, 2, P], F32, name="junk", tag="junk")
                nc.scalar.activation(out=junk[:], in_=of_two_blocks(s, ob), func=(ACT.Identity, ACT.Square)[kind],
                                     bias=neg_pivot[:, ob:ob + 1], scale=1.0,
                                     accum_out=msums[:, kind, ob, s // 2:s // 2 + 1])

        def second_piece():
            quant_y(1)
            move_y(1)
            after_moves = keep.tile([P, 1], I32, name="after_moves")
            nc.gpsimd.tensor_copy(out=after_moves[:], in_=scale_rows[2][:, 2 + PIECES[1][0], 0:1])

        def nothing():
            return None

        g_c1 = weight_copies(W_C1)
        haar_on_vector(0, (0, 1))
        quant_w(W_C1, g_c1)
        nc.vector.tensor_copy(out=bias_full[:], in_=bias_bf[:].unsqueeze(1).to_broadcast([P, ROW, 4]))
        haar_from_pe(0)
        quant_ll(0)
        g_q = weight_copies(W_Q)
        quant_w_half(W_Q, g_q, 0)
        add_bias(0)
        add_bias(1)
        quant_w_half(W_Q, g_q, 1)
        g_k = weight_copies(W_K)
        quant_y(0)
        g_kn = main.tile([P, 2048], BF16, name="grouped_neg", tag="grouped", bufs=2, align_bytes=64)
        nc.vector.tensor_scalar(out=g_kn[:, 0:1024], in0=g_k[:, 0:1024], scalar1=-1.0, scalar2=None, op0=ALU.mult)
        nc.scalar.activation(out=g_kn[:, 1024:2048], in_=g_k[:, 1024:2048], func=ACT.Copy, scale=-1.0)
        quant_w_half(W_K, g_k, 0)
        turn_middle()
        quant_w_half(W_KN, g_kn, 0)
        quant_w_half(W_K, g_k, 1)
        move_y(0)
        quant_w_half(W_KN, g_kn, 1)
        q_copy(0)
        haar_from_pe(1)


        after_head = keep.tile([P, 1], I32, name="after_head")
        nc.gpsimd.tensor_copy(out=after_head[:], in_=w_codes[W_KN][:, 511:512])
        def in_waits(s, part):
            if s in (4, 5):
                moments(0, 4 * (s - 4) + 2 * part, 4 * (s - 4) + 2 * part + 2)
            elif s == 6:
                moments(2, 2 * part, 2 * part + 2)

        haar_on_vector(1, (2, 3), True)
        first_scores()
        scores(0, 2, AHEAD)
        for s in range(STEPS):
            scores(s, AHEAD, scores_of(s))
            if ok(s - 3):
                divide(s - 3, 3 if s < STEPS - 1 else 4)
            if s == 1:
                late_sums = haar_by_reduce(2, 2)
            if s >= 4 and ok(s + 1):
                q_copy(s + 1)
            if ok(s - 1):
                exps(s - 1, 0)
            if s == 2:
                lay_out()
            if s == 0:
                q_copy(1)
            if s == 1:
                turn_copies(1, (1,))
                haar_from_turned(0)
                turn_copies(3, (1,))
                haar_from_turned(1)
                halve(2, 2, late_sums[:])
                haar_from_turned(3, 2)
            if s == STEPS - 1:
                moments(2, 4, 8)
            if ok(s - 2):
                weigh(s - 2, 0, 3)
            if SHARED_FROM <= s and s + 1 < LAST:
                scores_inwards(s)
            if ok(s - 2):
                weigh(s - 2, 3, 12)
            if s == 2:
                quant_y(2)
            if s == 0:
                g_v = weight_copies(W_V)
                quant_ll(1)
                add_bias_on_scalar(1)()
                tree_in_halves(s, lambda: quant_w(W_V, g_v), 0, None, second_piece)
            elif s == 1:
                tree_in_halves(s, nothing, 0, lambda: quant_ll(2))
                scores(s + 1, 0, AHEAD)
            else:
                tree_in_halves(s, (lambda: move_y(2)) if s == 2 else nothing, LAST_ON_VECTOR if s == STEPS - 1 else 0)
                if s == 2:
                    exps(1, 1)
                if ok(s + 1):
                    scores(s + 1, 0, AHEAD)
            if s == 0:
                turn_copies(0, (0, 1))
                turn_copies(1, (0,))
                pump_to(("h", 2, 3))
                halve(2, 3, banks[("h", 2, 3)][:, 0:256], 0, 2)
                scores(1, 0, AHEAD)
            if s == 1:
                exps(0, 1)
                lay_out = add_bias_on_scalar(2)
            elif ok(s - 1) and s != 2:
                if s == STEPS - 1:
                    pump_to(("F", s - 2, 35))
                    den_5 = main.tile([P, 4, P], F32, name="den_5", tag="lg", bufs=4)
                    nc.scalar.copy(out=den_5[:], in_=dens[s - 2][:])
                in_waits(s, 0)
                if s - 1 not in IN_TWO:
                    exps(s - 1, 1)
                in_waits(s, 1)
                if s - 1 in IN_TWO:
                    if s < STEPS - 1:
                        one_over_den(s - 2)
                    exps(s - 1, 1)
                if s - 1 not in IN_TWO:
                    exps(s - 1, 2)
            if ok(s - 2) and s < STEPS - 1 and (s == 2 or s - 1 not in IN_TWO):
                one_over_den(s - 2)
            if s == 3:
                nc.scalar.activation(out=neg_pivot[:], in_=att_rows[:, :, 7, 0], func=ACT.Copy, scale=-1.0)
                nc.scalar.activation(out=one_minus_a[:], in_=a_bf[:], func=ACT.Identity, bias=1.0, scale=-1.0)
                nc.scalar.activation(out=gam_f[:], in_=gam_bf[:], func=ACT.Copy, scale=-1.0)
                nc.scalar.activation(out=gam_p[:], in_=gam_bf[:], func=ACT.Copy, scale=1.0)
                nc.scalar.activation(out=neg_beta[:], in_=bet_bf[:], func=ACT.Copy, scale=-1.0)
        z_last = zs[STEPS - 1]
        for g0, g1 in LAST_GROUPS[1:]:
            nc.gpsimd.tensor_tensor(out=z_last[:, g0:g1, :], in0=z_last[:, g0:g1, :],
                                    in1=ms[LAST][:].unsqueeze(1).to_broadcast([P, g1 - g0, 512]), op=ALU.subtract)
        exps(STEPS - 1, 0)
        weigh(STEPS - 2, 0, 4)
        ev_sum = main.tile([P, 3, 512], F32, name="ev_sum", tag="t1", bufs=1)
        ev_sums.append(ev_sum)
        ev6 = evs[STEPS - 2]
        nc.gpsimd.tensor_tensor(out=ev_sum[:], in0=ev6[:, 0:3, :], in1=ev6[:, 3:6, :], op=ALU.add)
        weigh(STEPS - 2, 4, 6)
        exps(STEPS - 1, 1)
        lg_5 = main.tile([P, 4, P], F32, name="lg_5", tag="lg", bufs=4)
        nc.scalar.activation(out=lg_5[:], in_=den_5[:], func=ACT.Abs_reciprocal_sqrt)
        lgs[STEPS - 3] = lg_5
        log_den(STEPS - 2)
        exp_minus_log(STEPS - 3)
        weigh(STEPS - 1, 0, 6)
        log_den(STEPS - 1)
        exp_minus_log(STEPS - 2)
        exp_minus_log(STEPS - 1)
        for ob in range(4):
            block_stats(STEPS - 4, ob)
        first_part()
        divide(STEPS - 3)

        mean_var = keep.tile([P, 4, 2], F32, name="mean_var")
        gam_mean = keep.tile([P, 4], F32, name="gam_mean")
        rstd = keep.tile([P, 4], F32, name="rstd")
        gain = keep.tile([P, 4], F32, name="gain")
        shift = keep.tile([P, 4], F32, name="shift")
        out_v = out.rearrange("b (c r) h w -> c r b (h w)", r=4)
        ns = {}
        negs = {}
        ress = {}

        def col(t, ob):
            return t[:, ob:ob + 1]

        def divide_block(s, ob):
            pump_to(("G", s, 6 * ob + 5))
            nc.vector.tensor_tensor(out=att_rows[:, ob, 7 - s:9 + s:2 * s + 1, :], in0=nums[(s, ob)][:].rearrange("p (h f) -> p h f", h=2),
                                    in1=rds[s][:, ob, :].rearrange("p (h f) -> p h f", h=2), op=ALU.mult)

        def mean_and_var(ob):
            nc.vector.bn_aggr(out=mean_var[:, ob, :], in_=bn_parts[:, ob].rearrange("p g i -> p (g i)"))

        def statistics(ob):
            nc.vector.tensor_scalar(out=col(gam_mean, ob), in0=mean_var[:, ob, 0:1], scalar1=col(gam_p, ob), scalar2=None, op0=ALU.mult)
            nc.scalar.activation(out=col(rstd, ob), in_=mean_var[:, ob, 1:2], func=ACT.Abs_reciprocal_sqrt, bias=BN_EPS, scale=1.0)
            nc.scalar.activation(out=col(gain, ob), in_=col(rstd, ob), func=ACT.Identity, scale=col(gam_f, ob))
            nc.scalar.activation(out=col(shift, ob), in_=col(rstd, ob), func=ACT.Identity, bias=col(neg_beta, ob),
                                 scale=col(gam_mean, ob))

        def normalise(ob):
            if ob < 3:
                n = main.tile([P, NPIX], F32, name="n", tag="z", bufs=3, align_bytes=256)
            else:
                n = main.tile([P, NPIX], F32, name="n_last", tag="ev", bufs=2, align_bytes=256)
            ns[ob] = n

        def normalise_images(ob, b0, b1):
            nc.scalar.activation(out=ns[ob][:].rearrange("p (b y x) -> p b y x", b=NB, x=16)[:, b0:b1],
                                 in_=att[:, ob, :].rearrange("p (y b x) -> p b y x", b=NB, x=16)[:, b0:b1],
                                 func=ACT.Identity, bias=col(shift, ob), scale=col(gain, ob))

        def minus_part(ob):
            neg = main.tile([P, NPIX], F32, name="neg", tag=("t1", "t2")[ob % 2], bufs=1)
            nc.scalar.activation(out=neg[:].rearrange("p (b y x) -> p b y x", b=NB, x=16),
                                 in_=att[:, ob, :].rearrange("p (y b x) -> p b y x", b=NB, x=16),
                                 func=ACT.Relu, bias=col(shift, ob), scale=col(gain, ob))
            negs[ob] = neg

        def minus_part_on_vector(ob):
            neg = main.tile([P, NPIX], F32, name="neg_v", tag=("t1", "t2")[ob % 2], bufs=1)
            nc.vector.tensor_scalar(out=neg[:], in0=ns[ob][:], scalar1=0.0, scalar2=None, op0=ALU.max)
            negs[ob] = neg

        def normalise_on_vector(ob, b0=0, b1=NB):
            nc.vector.tensor_scalar(out=ns[ob][:].rearrange("p (b y x) -> p b y x", b=NB, x=16)[:, b0:b1],
                                    in0=att[:, ob, :].rearrange("p (y b x) -> p b y x", b=NB, x=16)[:, b0:b1],
                                    scalar1=col(gain, ob), scalar2=col(shift, ob), op0=ALU.mult, op1=ALU.add)

        def last_parts():
            neg = main.tile([P, NPIX], F32, name="neg_last", tag="t2", bufs=1)
            negs[3] = neg
            half = NPIX // 2
            normalise_images(3, 0, 2)
            nc.scalar.activation(out=neg[:, 0:half], in_=ns[3][:, 0:half], func=ACT.Relu)
            nc.scalar.activation(out=neg[:, half:].rearrange("p (b y x) -> p b y x", b=2, x=16),
                                 in_=att[:, 3, :].rearrange("p (y b x) -> p b y x", b=NB, x=16)[:, 2:4],
                                 func=ACT.Relu, bias=col(shift, 3), scale=col(gain, 3))

        def prelu_and_store(ob, b0=0, b1=NB):
            if b0 == 0:
                res = mid.tile([P, NPIX], F32, name="res", tag=("ll", "y_mid", "res_c", "res_d")[ob], align_bytes=64)
                ress[ob] = res
            res = ress[ob]
            images = slice(ROW * 4 * b0, ROW * 4 * b1)
            nc.vector.scalar_tensor_tensor(out=res[:, images], in0=negs[ob][:, images], scalar=one_minus_a[:, 0:1], in1=ns[ob][:, images],
                                           op0=ALU.mult, op1=ALU.subtract)
            nc.sync.dma_start(out=out_v[:, ob, b0:b1], in_=res[:].rearrange("p (b f) -> p b f", b=NB)[:, b0:b1])

        B5 = STEPS - 3
        B6 = STEPS - 2
        B7 = STEPS - 1
        block_stats(B5, 0)
        divide_block(B6, 0)
        block_stats(B5, 1)
        divide_block(B6, 1)
        block_stats(B5, 2)
        divide_block(B6, 2)
        block_stats(B5, 3)
        nc.vector.tensor_copy(out=bn_parts[:, :, 0, 1:3], in_=first_four[:])
        divide_block(B7, 0)
        divide_block(B7, 1)
        block_stats(B6, 0)
        divide_block(B7, 2)
        mean_and_var(0)
        block_stats(B6, 1)
        statistics(0)
        normalise(0)
        minus_part(0)
        divide_block(B6, 3)
        mean_and_var(1)
        divide_block(B7, 3)
        normalise_on_vector(0)
        statistics(1)
        normalise(1)
        minus_part(1)
        block_stats(B6, 2)
        block_stats(B6, 3)
        mean_and_var(2)
        mean_and_var(3)
        prelu_and_store(0)
        statistics(2)
        normalise(2)
        statistics(3)
        minus_part(2)
        normalise_on_vector(1)
        prelu_and_store(1)
        normalise_on_vector(2)
        normalise(3)
        last_parts()
        normalise_on_vector(3, 2, 4)
        prelu_and_store(2)
        prelu_and_store(3, 0, 2)
        prelu_and_store(3, 2, 4)
